import numpy as np
import ml_dtypes


def mxq(x, axis, fmt="e4m3"):
    dtype, down = {"e4m3": (ml_dtypes.float8_e4m3fn, 7), "e5m2": (ml_dtypes.float8_e5m2, 14)}[fmt]
    v = np.moveaxis(np.asarray(x, np.float32).astype(ml_dtypes.bfloat16).astype(np.float64), axis, -1)
    blocks = v.reshape(v.shape[:-1] + (-1, 32))
    amax = np.abs(blocks).max(-1, keepdims=True)
    byte = np.maximum(np.where(amax > 0, np.frexp(amax)[1] - 1 + 127, 0) - down, 1)
    scale = np.exp2(byte - 127.0)
    codes = (blocks / scale).astype(np.float32).astype(dtype).astype(np.float64)
    return np.moveaxis((codes * scale).reshape(v.shape), -1, axis)


WIDE = False


def mx_kscale(k):
    if not WIDE:
        return np.ones(k)
    levels = np.array([10, -10, 5, -5, 0])
    if k % 512:
        return np.exp2(np.random.permutation(np.resize(levels, k // 32))).repeat(32)
    a = np.empty((k // 512, 16))
    for p in range(k // 512):
        a[p, :8] = np.random.permutation(np.resize(levels, 8))
        for g in range(8):
            far = levels[np.abs(levels - a[p, g]) >= 10]
            a[p, g + 8] = far[np.random.randint(len(far))]
    return np.exp2(a.ravel()).repeat(32)


BF16 = ml_dtypes.bfloat16


def bf(x):
    return np.asarray(x, np.float32).astype(BF16)


def f64(x):
    return np.asarray(x).astype(np.float64)


B, S, A, O, H, L = 1024, 1024, 128, 1920, 1024, 384
K1 = S + A + O


def draw0():
    s = mx_kscale(K1)
    t = mx_kscale(H)
    col = np.concatenate([np.full(L, 0.7), np.full(L, 0.14)]) / np.sqrt(H)
    return {"prev_state": bf(np.random.standard_normal((B, S)) * s[:S]),
            "prev_action": bf(np.random.standard_normal((B, A)) * s[S:S + A]),
            "observation": bf(np.random.standard_normal((B, O)) * s[S + A:]),
            "eps": bf(np.random.standard_normal((B, L))),
            "rep_W1": bf(np.random.standard_normal((K1, H)) / np.sqrt(K1) / s[:, None] * t),
            "rep_b1": bf(np.random.standard_normal(H) * 0.1 * t),
            "rep_W2": bf(np.random.standard_normal((H, 2 * L)) * col / t[:, None]),
            "rep_b2": bf(np.concatenate([0.1 * np.random.standard_normal(L), 1.0 + 0.1 * np.random.standard_normal(L)]))}


def core(prev_state, prev_action, observation, eps, rep_W1, rep_b1, rep_W2, rep_b2):
    x = np.concatenate([f64(prev_state), f64(prev_action), f64(observation)], axis=-1)
    h1 = np.maximum((mxq(x, 1, "e4m3") @ mxq(f64(rep_W1), 0, "e4m3")) + f64(rep_b1), 0.0)
    out = (mxq(h1, 1, "e4m3") @ mxq(f64(rep_W2), 0, "e4m3")) + f64(rep_b2)
    mean, std = np.split(out, 2, axis=-1)
    sample = mean + np.sqrt(std) * f64(eps)
    return mean, std, sample


def e4m3fn_bytes(y):
    return np.clip(np.asarray(y, np.float64), -448.0, 448.0).astype(np.float32).astype(ml_dtypes.float8_e4m3fn).view(np.uint8)


def e4m3fn_values(b):
    return np.asarray(b, np.uint8).view(ml_dtypes.float8_e4m3fn).astype(np.float64)


def setup_inputs():
    d = draw0()
    x0 = np.asarray(d['observation']).astype(np.float64)
    s = (np.max(np.abs(x0), axis=(0,), keepdims=True) / 448.0).astype(np.float32)
    out = {}
    for k, v in d.items():
        if k == 'observation':
            out['observation_bytes'] = e4m3fn_bytes(x0 / s.astype(np.float64))
            out['observation_scale'] = s
        else:
            out[k] = v
    return out


def reference(prev_state, prev_action, observation_bytes, observation_scale, eps, rep_W1, rep_b1, rep_W2, rep_b2):
    return core(prev_state, prev_action, e4m3fn_values(observation_bytes) * observation_scale.astype(np.float64), eps, rep_W1, rep_b1, rep_W2, rep_b2)

@@ -1,0 +1,550 @@
+from contextlib import ExitStack
+
+import concourse.mybir as mybir
+from concourse.masks import make_identity
+
+B, S, A, O, H, L = 1024, 1024, 128, 1920, 1024, 384
+K1 = S + A + O
+FLOPS = 2 * B * K1 * H + 2 * B * H * 2 * L
+
+F32 = mybir.dt.float32
+BF16 = mybir.dt.bfloat16
+U32 = mybir.dt.uint32
+U8 = mybir.dt.uint8
+FP8 = mybir.dt.float8_e4m3fn
+FP8X4 = mybir.dt.float8_e4m3fn_x4
+ACT = mybir.ActivationFunctionType
+ALU = mybir.AluOpType
+
+P = 128
+G1 = K1 // 512
+G2 = H // 512
+NT = B // P
+
+
+def tile_rssm_pa_kernel(tc, prev_state, prev_action, obs_bytes, obs_scale, eps,
+                                    w1, b1, w2, b2, out_mean, out_std, out_sample):
+    nc = tc.nc
+
+    state_v = prev_state.rearrange("(p i) k -> p i k", i=NT)
+    action_v = prev_action.rearrange("(p i) k -> p i k", i=NT)
+    bytes_v = obs_bytes.rearrange("(p i) k -> p i k", i=NT)
+    eps_v = eps.rearrange("(p i) n -> p i n", i=NT)
+    mean_v = out_mean.rearrange("(p i) n -> p i n", i=NT)
+    std_v = out_std.rearrange("(p i) n -> p i n", i=NT)
+    sample_v = out_sample.rearrange("(p i) n -> p i n", i=NT)
+    w1_v = w1.rearrange("(g p j) c -> g p j c", p=P, j=4)
+    w2_v = w2.rearrange("(g p j) c -> g p j c", p=P, j=4)
+
+    with ExitStack() as ctx:
+        keep = ctx.enter_context(tc.tile_pool(name="keep", bufs=1))
+        rows = ctx.enter_context(tc.tile_pool(name="rows", bufs=3))
+        raw = ctx.enter_context(tc.tile_pool(name="raw", bufs=7))
+        inter = ctx.enter_context(tc.tile_pool(name="inter", bufs=8))
+        hid = ctx.enter_context(tc.tile_pool(name="hid", bufs=2))
+        outp = ctx.enter_context(tc.tile_pool(name="outp", bufs=2))
+        psum = ctx.enter_context(tc.psum_pool(name="psum", bufs=4))
+
+        ident = keep.tile([P, P], F32)
+        make_identity(nc, ident[:])
+        warm = keep.tile([P, 1], F32)
+        nc.vector.memset(warm[:], 1.0)
+        nc.scalar.activation(warm[:], warm[:], ACT.Sqrt)
+
+        w1c = keep.tile([P, G1, H], U32, align_bytes=64)
+        w1s = keep.tile([P, G1, H], U8, align_bytes=64)
+        w2c = keep.tile([P, G2, 2 * L], U32, align_bytes=64)
+        w2s = keep.tile([P, G2, 2 * L], U8, align_bytes=64)
+        scale = keep.tile([P, O], F32)
+        b1c = keep.tile([P, G2, 4], BF16)
+        b2b = keep.tile([P, 2 * L], BF16)
+        eps_sb = keep.tile([P, NT, L], BF16)
+
+        xr = {}
+        ob = {}
+        w1r = {}
+
+        def load_w1(half, g):
+            t = raw.tile([P, 4, 512], BF16, name="w1r")
+            nc.sync.dma_start(out=t[:], in_=w1_v[g][:, :, 512 * half:512 * half + 512])
+            w1r[half, g] = t
+
+        def new_rows(q):
+            xr[q] = rows.tile([P, 2, K1], BF16, name="xr", align_bytes=64)
+
+        def load_state(q, g0, g1):
+            nc.sync.dma_start(out=xr[q][:, :, 512 * g0:512 * g1],
+                              in_=state_v[:, 2 * q:2 * q + 2, 512 * g0:512 * g1])
+
+        def load_obs(q):
+            t = rows.tile([P, 2, O], U8, name="ob")
+            nc.sync.dma_start(out=t[:], in_=bytes_v[:, 2 * q:2 * q + 2, :])
+            ob[q] = t
+            nc.sync.dma_start(out=xr[q][:, :, S:S + A], in_=action_v[:, 2 * q:2 * q + 2, :])
+
+        def product(q, i, c0, c1):
+            nc.vector.tensor_tensor(out=xr[q][:, i, S + A + c0:S + A + c1],
+                                    in0=ob[q][:, i, c0:c1].bitcast(FP8),
+                                    in1=scale[:, c0:c1], op=ALU.mult)
+
+        def interleave_w1(half, g, engine):
+            t = inter.tile([P, 2048], BF16, name="il", align_bytes=64)
+            dst = t[:].rearrange("p (t m j) -> p m j t", t=4, j=4)
+            src = w1r[half, g][:].rearrange("p j (m t) -> p m j t", t=4)
+            engine(out=dst, in_=src)
+            return t
+
+        def quant_w1(half, g, t):
+            nc.vector.quantize_mx(out=w1c[:, g, 512 * half:512 * half + 512].bitcast(FP8X4),
+                                  scales=w1s[:, g, 512 * half:512 * half + 512], in_=t[:])
+
+        class_blocks = [[0, 1], [2], [3]]
+        xc = {}
+        xs = {}
+        hc = {}
+        hs = {}
+        hp = {}
+        for b, qs in enumerate(class_blocks):
+            n = 256 * len(qs)
+            xc[b] = keep.tile([P, G1, n], U32, name="xc%d" % b, align_bytes=64)
+            xs[b] = keep.tile([P, G1, n], U8, name="xs%d" % b, align_bytes=64)
+            hc[b] = keep.tile([P, G2, n], U32, name="hc%d" % b, align_bytes=64)
+            hs[b] = keep.tile([P, G2, n], U8, name="hs%d" % b, align_bytes=64)
+
+        def x_prep(b, gs):
+            t = inter.tile([P, 2048], BF16, name="il", align_bytes=64)
+            words_out = t[:].bitcast(F32)
+            units = [(g, q) for g in gs for q in class_blocks[b]]
+            for h, (g, q) in enumerate(units):
+                tp = psum.tile([P, 2, 256], F32, name="tp")
+                for i in range(2):
+                    words = xr[q][:, i, :].bitcast(F32)
+                    for u in range(2):
+                        nc.tensor.transpose(tp[:, u, 128 * i:128 * i + 128],
+                                            words[:, 256 * g + u:256 * g + 256:2], ident[:])
+                dst = words_out[:, 512 * h:512 * h + 512].rearrange("p (r u) -> p r u", u=2)
+                nc.scalar.copy(out=dst, in_=tp[:].rearrange("p u r -> p r u"))
+            nc.vector.quantize_mx(out=xc[b][:, gs[0]:gs[-1] + 1, :].rearrange("p g n -> p (g n)").bitcast(FP8X4),
+                                  scales=xs[b][:, gs[0]:gs[-1] + 1, :].rearrange("p g n -> p (g n)"), in_=t[:])
+
+        def mm1(acc, b, half, t, g):
+            c0 = 512 * half + 128 * t
+            n = 256 * len(class_blocks[b])
+            nc.tensor.matmul_mx(out=acc[:, :n],
+                                lhsT=w1c[:, g, c0:c0 + 128].bitcast(FP8X4),
+                                lhsT_scale=w1s[:, g, c0:c0 + 128],
+                                rhs=xc[b][:, g, :].bitcast(FP8X4),
+                                rhs_scale=xs[b][:, g, :],
+                                start=(g == 0), stop=(g == G1 - 1))
+
+        def new_accs():
+            return [psum.tile([P, 512], F32, name="acc") for t in range(4)]
+
+        def relu(acc, b, half, t):
+            n = 256 * len(class_blocks[b])
+            if t == 0:
+                hp[b, half] = hid.tile([P, 4, 512], BF16, name="hp")
+            nc.scalar.activation(hp[b, half][:, t, :n], acc[:, :n], ACT.Relu, bias=b1c[:, half, t:t + 1])
+
+        def h_prep(b, half, engine):
+            n = 256 * len(class_blocks[b])
+            t = inter.tile([P, 2048], BF16, name="il", align_bytes=64)
+            engine(out=t[:, :4 * n].rearrange("p (c i t) -> p c t i", i=4, t=4),
+                   in_=hp[b, half][:, :, :n].rearrange("p t (c i) -> p c t i", i=4))
+            nc.vector.quantize_mx(out=hc[b][:, half, :].bitcast(FP8X4), scales=hs[b][:, half, :], in_=t[:, :4 * n])
+
+        w2r = {}
+
+        def load_w2(g):
+            for c0, c1 in ((0, 512), (512, 768)):
+                t = raw.tile([P, 4, c1 - c0], BF16, name="w1r")
+                nc.sync.dma_start(out=t[:], in_=w2_v[g][:, :, c0:c1])
+                w2r[g, c0] = t
+
+        def w2_prep(g, engine):
+            for c0, c1 in ((0, 512), (512, 768)):
+                t = inter.tile([P, 2048], BF16, name="il", align_bytes=64)
+                n = 4 * (c1 - c0)
+                engine(out=t[:, :n].rearrange("p (c i j) -> p c j i", i=4, j=4),
+                       in_=w2r[g, c0][:].rearrange("p j (c i) -> p c j i", i=4))
+                nc.vector.quantize_mx(out=w2c[:, g, c0:c1].bitcast(FP8X4), scales=w2s[:, g, c0:c1], in_=t[:, :n])
+
+        def stage2(b, q, split):
+            h = class_blocks[b].index(q)
+            mean_sb = outp.tile([P, 2, L], F32, name="mean_sb")
+            std_sb = outp.tile([P, 2, L], F32, name="std_sb")
+            smp = outp.tile([P, 2, L], F32, name="smp")
+
+            def sample(s):
+                nc.scalar.activation(smp[:, s, :], std_sb[:, s, :], ACT.Sqrt)
+                nc.vector.tensor_mul(out=smp[:, s, :], in0=smp[:, s, :], in1=eps_sb[:, 2 * q + s.start:2 * q + s.stop, :])
+                nc.vector.tensor_add(out=smp[:, s, :], in0=smp[:, s, :], in1=mean_sb[:, s, :])
+
+            for i in range(2):
+                r0 = 256 * h + 128 * i
+                for part in (1, 0):
+                    ps = psum.tile([P, 512], F32, name="tp")
+                    for c0, c1 in ((0, 256), (256, 384)):
+                        w0, w1_ = L * part + c0, L * part + c1
+                        for g in range(G2):
+                            nc.tensor.matmul_mx(out=ps[:, c0:c1],
+                                                lhsT=hc[b][:, g, r0:r0 + 128].bitcast(FP8X4),
+                                                lhsT_scale=hs[b][:, g, r0:r0 + 128],
+                                                rhs=w2c[:, g, w0:w1_].bitcast(FP8X4),
+                                                rhs_scale=w2s[:, g, w0:w1_],
+                                                start=(g == 0), stop=(g == G2 - 1))
+                    dst = std_sb if part else mean_sb
+                    nc.vector.tensor_add(out=dst[:, i, :], in0=ps[:, :L], in1=b2b[:, L * part:L * part + L])
+                if split:
+                    sample(slice(i, i + 1))
+            if not split:
+                sample(slice(0, 2))
+            nc.sync.dma_start(out=std_v[:, 2 * q:2 * q + 2, :], in_=std_sb[:])
+            nc.sync.dma_start(out=mean_v[:, 2 * q:2 * q + 2, :], in_=mean_sb[:])
+            nc.sync.dma_start(out=sample_v[:, 2 * q:2 * q + 2, :], in_=smp[:])
+
+        srow = keep.tile([P, P], F32)
+        nc.gpsimd.memset(srow[:], 0.0)
+        nc.sync.dma_start(out=srow[:15, :], in_=obs_scale.rearrange("o (c k) -> (o c) k", k=P))
+        scol = keep.tile([P, 16], F32)
+        tp = psum.tile([P, 512], F32, name="tp")
+        nc.tensor.transpose(tp[:, :P], srow[:], ident[:])
+        nc.scalar.copy(out=scol[:], in_=tp[:, :16])
+        for c0 in range(0, 15, 4):
+            c1 = min(c0 + 4, 15)
+            tp = psum.tile([P, 512], F32, name="tp")
+            for c in range(c0, c1):
+                nc.tensor.transpose(tp[:, P * (c - c0):P * (c - c0 + 1)], scol[:, c:c + 1].to_broadcast([P, P]), ident[:])
+            copy = nc.vector.tensor_copy if "SVSS"[c0 // 4] == "V" else nc.scalar.copy
+            copy(out=scale[:, P * c0:P * c1], in_=tp[:, :P * (c1 - c0)])
+
+        new_rows(0)
+        new_rows(1)
+        load_w1(0, 0)
+        load_obs(0)
+        load_state(0, 0, 1)
+        load_state(1, 0, 1)
+        load_w1(0, 1)
+        load_obs(1)
+        load_state(0, 1, 2)
+        load_state(1, 1, 2)
+        for g in range(2, 6):
+            load_w1(0, g)
+        nc.sync.dma_start(out=b1c[:], in_=b1.rearrange("(g p t) -> p g t", p=P, t=4))
+        load_w1(1, 0)
+
+        load_w1(1, 1)
+        new_rows(2)
+        load_obs(2)
+        load_state(2, 0, 2)
+        load_w1(1, 2)
+        load_w1(1, 3)
+        new_rows(3)
+        load_obs(3)
+        load_state(3, 0, 2)
+        load_w1(1, 4)
+        load_w1(1, 5)
+        load_w2(0)
+        load_w2(1)
+        nc.sync.dma_start(out=b2b[:], in_=b2.partition_broadcast(P))
+        nc.sync.dma_start(out=eps_sb[:], in_=eps_v)
+
+        vec, sca = nc.vector.tensor_copy, nc.scalar.copy
+        units = [(0, [g]) for g in range(6)] + [(1, [0, 1]), (1, [2, 3]), (1, [4, 5]), (2, [0, 1]), (2, [2, 3]), (2, [4, 5])]
+        tps, wi, xi, accs, hi, w2i, ps, ep = {}, {}, {}, {}, {}, {}, {}, {}
+        ENG = {"V": vec, "S": sca}
+
+        def il(n):
+            wi[n] = interleave_w1(n // 6, n % 6, ENG["VSSSSVSSVVSV"[n]])
+
+        def wq(n):
+            quant_w1(n // 6, n % 6, wi[n])
+
+        def T(u):
+            b, gs = units[u]
+            tps[u] = []
+            for g in gs:
+                for q in class_blocks[b]:
+                    tp = psum.tile([P, 2, 256], F32, name="tp")
+                    for i in range(2):
+                        words = xr[q][:, i, :].bitcast(F32)
+                        for w in range(2):
+                            nc.tensor.transpose(tp[:, w, 128 * i:128 * i + 128],
+                                                words[:, 256 * g + w:256 * g + 256:2], ident[:])
+                    tps[u].append(tp)
+
+        def Cx(u):
+            t = inter.tile([P, 2048], BF16, name="il", align_bytes=64)
+            for h, tp in enumerate(tps[u]):
+                nc.scalar.copy(out=t[:].bitcast(F32)[:, 512 * h:512 * h + 512].rearrange("p (r u) -> p r u", u=2),
+                               in_=tp[:].rearrange("p u r -> p r u"))
+            xi[u] = t
+
+        def Q(u):
+            b, gs = units[u]
+            nc.vector.quantize_mx(out=xc[b][:, gs[0]:gs[-1] + 1, :].rearrange("p g n -> p (g n)").bitcast(FP8X4),
+                                  scales=xs[b][:, gs[0]:gs[-1] + 1, :].rearrange("p g n -> p (g n)"), in_=xi[u][:])
+
+        def PR(k):
+            if k < 8:
+                product((k // 2) % 2, k % 2, 0 if k < 4 else 896, 896 if k < 4 else O)
+            else:
+                product(2 + (k - 8) // 2, k % 2, 0, O)
+
+        def M(b, half, g):
+            if g == 0:
+                accs[b, half] = new_accs()
+            for tt in range(4):
+                mm1(accs[b, half][tt], b, half, tt, g)
+
+        def R(b, half):
+            for tt in range(4):
+                relu(accs[b, half][tt], b, half, tt)
+
+        def C1(b, half, tt):
+            acc = psum.tile([P, 512], F32, name="acc")
+            for g in range(G1):
+                mm1(acc, b, half, tt, g)
+            accs[b, half, tt] = acc
+
+        def R1(b, half, tt):
+            relu(accs[b, half, tt], b, half, tt)
+
+        def HI(b, half):
+            n = 256 * len(class_blocks[b])
+            t = inter.tile([P, 2048], BF16, name="il", align_bytes=64)
+            ENG[["SS","SS","SS"][b][half]](
+                out=t[:, :4 * n].rearrange("p (c i t) -> p c t i", i=4, t=4),
+                in_=hp[b, half][:, :, :n].rearrange("p t (c i) -> p c t i", i=4))
+            hi[b, half] = t
+
+        def HQ(b, half):
+            n = 256 * len(class_blocks[b])
+            nc.vector.quantize_mx(out=hc[b][:, half, :].bitcast(FP8X4), scales=hs[b][:, half, :], in_=hi[b, half][:, :4 * n])
+
+        def W2RANGE(k):
+            return k // 2, 512 * (k % 2), 512 + 256 * (k % 2)
+
+        def WI(k):
+            g, c0, c1 = W2RANGE(k)
+            t = inter.tile([P, 2048], BF16, name="il", align_bytes=64)
+            ENG["VVVS"[k]](out=t[:, :4 * (c1 - c0)].rearrange("p (c i j) -> p c j i", i=4, j=4),
+                               in_=w2r[g, c0][:].rearrange("p j (c i) -> p c j i", i=4))
+            w2i[k] = t
+
+        def WQ(k):
+            g, c0, c1 = W2RANGE(k)
+            nc.vector.quantize_mx(out=w2c[:, g, c0:c1].bitcast(FP8X4), scales=w2s[:, g, c0:c1], in_=w2i[k][:, :4 * (c1 - c0)])
+
+        def S2(q, i):
+            b = 0 if q < 2 else q - 1
+            r0 = 256 * class_blocks[b].index(q) + 128 * i
+            for part in (1, 0):
+                acc = psum.tile([P, 512], F32, name="tp")
+                for c0, c1 in ((0, 256), (256, 384)):
+                    w0, w9 = L * part + c0, L * part + c1
+                    for g in range(G2):
+                        nc.tensor.matmul_mx(out=acc[:, c0:c1],
+                                            lhsT=hc[b][:, g, r0:r0 + 128].bitcast(FP8X4),
+                                            lhsT_scale=hs[b][:, g, r0:r0 + 128],
+                                            rhs=w2c[:, g, w0:w9].bitcast(FP8X4),
+                                            rhs_scale=w2s[:, g, w0:w9],
+                                            start=(g == 0), stop=(g == G2 - 1))
+                ps[q, i, part] = acc
+
+        def BA(q, i):
+            if q not in ep:
+                mean_sb = outp.tile([P, 2, L], F32, name="mean_sb")
+                std_sb = outp.tile([P, 2, L], F32, name="std_sb")
+                smp = outp.tile([P, 2, L], F32, name="smp")
+                ep[q] = (mean_sb, std_sb, smp)
+            for part in (1, 0):
+                nc.vector.tensor_add(out=ep[q][part][:, i, :], in0=ps[q, i, part][:, :L], in1=b2b[:, L * part:L * part + L])
+
+        def SQ(q, i):
+            nc.scalar.activation(ep[q][2][:, i[0]:i[-1] + 1, :], ep[q][1][:, i[0]:i[-1] + 1, :], ACT.Sqrt)
+
+        def MU(q, i):
+            s = ep[q][2][:, i[0]:i[-1] + 1, :]
+            nc.vector.tensor_mul(out=s, in0=s, in1=eps_sb[:, 2 * q + i[0]:2 * q + i[-1] + 1, :])
+
+        def AD(q, i):
+            s = ep[q][2][:, i[0]:i[-1] + 1, :]
+            nc.vector.tensor_add(out=s, in0=s, in1=ep[q][0][:, i[0]:i[-1] + 1, :])
+
+        def OUT(q):
+            for view, part in ((std_v, 1), (mean_v, 0), (sample_v, 2)):
+                nc.sync.dma_start(out=view[:, 2 * q:2 * q + 2, :], in_=ep[q][part][:])
+
+        with tc.manual_schedule(engines={mybir.EngineType.PE, mybir.EngineType.DVE, mybir.EngineType.Activation}):
+            il(0)
+            T(0)
+            PR(5)
+            PR(0)
+            PR(4)
+            Cx(0)
+            Q(0)
+            PR(1)
+            PR(2)
+            il(1)
+            T(1)
+            wq(0)
+            Cx(1)
+            Q(1)
+            il(2)
+            PR(3)
+            PR(7)
+            wq(1)
+            il(3)
+            il(5)
+            T(2)
+            wq(2)
+            Cx(2)
+            wq(5)
+            T(3)
+            PR(6)
+            Cx(3)
+            il(7)
+            T(4)
+            T(5)
+            il(4)
+            Cx(4)
+            wq(3)
+            Cx(5)
+            PR(9)
+            Q(2)
+            M(0, 0, 0)
+            il(6)
+            PR(8)
+            Q(3)
+            wq(4)
+            M(0, 0, 1)
+            il(8)
+            M(0, 0, 2)
+            Q(4)
+            Q(5)
+            il(11)
+            T(6)
+            Cx(6)
+            wq(7)
+            T(8)
+            M(0, 0, 3)
+            M(0, 0, 4)
+            il(9)
+            wq(6)
+            Cx(8)
+            M(0, 0, 5)
+            wq(11)
+            wq(9)
+            T(9)
+            T(7)
+            R(0, 0)
+            il(10)
+            HI(0, 0)
+            wq(8)
+            M(0, 1, 0)
+            Cx(7)
+            M(0, 1, 1)
+            wq(10)
+            PR(11)
+            M(0, 1, 2)
+            PR(10)
+            M(0, 1, 3)
+            Q(7)
+            Q(6)
+            Q(8)
+            M(0, 1, 4)
+            Cx(9)
+            M(0, 1, 5)
+            T(10)
+            T(11)
+            WI(0)
+            R(0, 1)
+            Cx(11)
+            HQ(0, 0)
+            HI(0, 1)
+            M(1, 0, 0)
+            M(1, 0, 1)
+            M(1, 0, 2)
+            M(1, 0, 3)
+            M(1, 0, 4)
+            WI(1)
+            WI(2)
+            WQ(0)
+            M(1, 0, 5)
+            R(1, 0)
+            HQ(0, 1)
+            C1(1, 1, 3)
+            WI(3)
+            WQ(1)
+            C1(1, 1, 0)
+            Cx(10)
+            R1(1, 1, 0)
+            C1(1, 1, 1)
+            WQ(2)
+            R1(1, 1, 1)
+            WQ(3)
+            C1(1, 1, 2)
+            S2(0, 1)
+            Q(9)
+            Q(11)
+            R1(1, 1, 2)
+            S2(0, 0)
+            BA(0, 1)
+            R1(1, 1, 3)
+            Q(10)
+            HI(1, 0)
+            BA(0, 0)
+            M(2, 0, 0)
+            S2(1, 0)
+            M(2, 0, 1)
+            SQ(0, (0,1))
+            BA(1, 0)
+            M(2, 0, 2)
+            HI(1, 1)
+            MU(0, (0,1))
+            AD(0, (0,1))
+            M(2, 0, 3)
+            M(2, 0, 4)
+            M(2, 0, 5)
+            S2(1, 1)
+            R(2, 0)
+            BA(1, 1)
+            C1(2, 1, 0)
+            OUT(0)
+            C1(2, 1, 1)
+            C1(2, 1, 2)
+            HQ(1, 1)
+            HQ(1, 0)
+            SQ(1, (0,1))
+            C1(2, 1, 3)
+            S2(2, 1)
+            MU(1, (0,1))
+            R1(2, 1, 0)
+            AD(1, (0,1))
+            OUT(1)
+            R1(2, 1, 1)
+            HI(2, 0)
+            HQ(2, 0)
+            BA(2, 1)
+            R1(2, 1, 2)
+            S2(2, 0)
+            R1(2, 1, 3)
+            BA(2, 0)
+            HI(2, 1)
+            SQ(2, (0,1))
+            HQ(2, 1)
+            S2(3, 1)
+            MU(2, (0,1))
+            BA(3, 1)
+            S2(3, 0)
+            BA(3, 0)
+            AD(2, (0,1))
+            OUT(2)
+            SQ(3, (0,))
+            MU(3, (0,))
+            SQ(3, (1,))
+            MU(3, (1,))
+            AD(3, (0,))
+            AD(3, (1,))
+            OUT(3)

@@ -20,10 +20,17 @@ P = 128
 G1 = K1 // 512
 G2 = H // 512
 NT = B // P
+NQ = NT // 2
+SCALE_ROWS = 16
+SCALE_COLS = O // SCALE_ROWS
+SHARE = (18, 32)
+LEAD = 3
+W2V = (1, 2, 3)
+HV = ((0, 0), (3, 1))
 
 
 def tile_rssm_pa_kernel(tc, prev_state, prev_action, obs_bytes, obs_scale, eps,
-                                    w1, b1, w2, b2, out_mean, out_std, out_sample):
+                                       w1, b1, w2, b2, out_mean, out_std, out_sample):
     nc = tc.nc
 
     state_v = prev_state.rearrange("(p i) k -> p i k", i=NT)
@@ -40,16 +47,11 @@ def tile_rssm_pa_kernel(tc, prev_state, prev_action, obs_bytes, obs_scale, eps,
         keep = ctx.enter_context(tc.tile_pool(name="keep", bufs=1))
         rows = ctx.enter_context(tc.tile_pool(name="rows", bufs=3))
         raw = ctx.enter_context(tc.tile_pool(name="raw", bufs=7))
-        inter = ctx.enter_context(tc.tile_pool(name="inter", bufs=8))
+        inter = ctx.enter_context(tc.tile_pool(name="inter", bufs=3))
         hid = ctx.enter_context(tc.tile_pool(name="hid", bufs=2))
-        outp = ctx.enter_context(tc.tile_pool(name="outp", bufs=2))
+        outp = ctx.enter_context(tc.tile_pool(name="outp", bufs=4))
         psum = ctx.enter_context(tc.psum_pool(name="psum", bufs=4))
-
-        ident = keep.tile([P, P], F32)
-        make_identity(nc, ident[:])
-        warm = keep.tile([P, 1], F32)
-        nc.vector.memset(warm[:], 1.0)
-        nc.scalar.activation(warm[:], warm[:], ACT.Sqrt)
+        ctx.enter_context(tc.manual_schedule())
 
         w1c = keep.tile([P, G1, H], U32, align_bytes=64)
         w1s = keep.tile([P, G1, H], U8, align_bytes=64)
@@ -59,492 +61,436 @@ def tile_rssm_pa_kernel(tc, prev_state, prev_action, obs_bytes, obs_scale, eps,
         b1c = keep.tile([P, G2, 4], BF16)
         b2b = keep.tile([P, 2 * L], BF16)
         eps_sb = keep.tile([P, NT, L], BF16)
-
-        xr = {}
-        ob = {}
-        w1r = {}
-
-        def load_w1(half, g):
-            t = raw.tile([P, 4, 512], BF16, name="w1r")
-            nc.sync.dma_start(out=t[:], in_=w1_v[g][:, :, 512 * half:512 * half + 512])
-            w1r[half, g] = t
-
-        def new_rows(q):
-            xr[q] = rows.tile([P, 2, K1], BF16, name="xr", align_bytes=64)
-
-        def load_state(q, g0, g1):
-            nc.sync.dma_start(out=xr[q][:, :, 512 * g0:512 * g1],
-                              in_=state_v[:, 2 * q:2 * q + 2, 512 * g0:512 * g1])
-
-        def load_obs(q):
-            t = rows.tile([P, 2, O], U8, name="ob")
-            nc.sync.dma_start(out=t[:], in_=bytes_v[:, 2 * q:2 * q + 2, :])
-            ob[q] = t
-            nc.sync.dma_start(out=xr[q][:, :, S:S + A], in_=action_v[:, 2 * q:2 * q + 2, :])
-
-        def product(q, i, c0, c1):
-            nc.vector.tensor_tensor(out=xr[q][:, i, S + A + c0:S + A + c1],
-                                    in0=ob[q][:, i, c0:c1].bitcast(FP8),
-                                    in1=scale[:, c0:c1], op=ALU.mult)
-
-        def interleave_w1(half, g, engine):
-            t = inter.tile([P, 2048], BF16, name="il", align_bytes=64)
-            dst = t[:].rearrange("p (t m j) -> p m j t", t=4, j=4)
-            src = w1r[half, g][:].rearrange("p j (m t) -> p m j t", t=4)
-            engine(out=dst, in_=src)
-            return t
-
-        def quant_w1(half, g, t):
-            nc.vector.quantize_mx(out=w1c[:, g, 512 * half:512 * half + 512].bitcast(FP8X4),
-                                  scales=w1s[:, g, 512 * half:512 * half + 512], in_=t[:])
-
-        class_blocks = [[0, 1], [2], [3]]
-        xc = {}
-        xs = {}
-        hc = {}
-        hs = {}
-        hp = {}
-        for b, qs in enumerate(class_blocks):
+        blocks = [[0, 1], [2], [3]]
+        xc, xs, hc, hs = {}, {}, {}, {}
+        for b, qs in enumerate(blocks):
             n = 256 * len(qs)
             xc[b] = keep.tile([P, G1, n], U32, name="xc%d" % b, align_bytes=64)
             xs[b] = keep.tile([P, G1, n], U8, name="xs%d" % b, align_bytes=64)
+        spans = [(0, 0, 512), (1, 0, 256), (2, 0, 128), (2, 128, 128)]
+        span_of = [0, 0, 0, 0, 1, 1, 2, 3]
+        first_tile = [0, 4, 6, 7]
+        for b, (xb, r0, n) in enumerate(spans):
             hc[b] = keep.tile([P, G2, n], U32, name="hc%d" % b, align_bytes=64)
             hs[b] = keep.tile([P, G2, n], U8, name="hs%d" % b, align_bytes=64)
 
-        def x_prep(b, gs):
-            t = inter.tile([P, 2048], BF16, name="il", align_bytes=64)
-            words_out = t[:].bitcast(F32)
-            units = [(g, q) for g in gs for q in class_blocks[b]]
-            for h, (g, q) in enumerate(units):
-                tp = psum.tile([P, 2, 256], F32, name="tp")
-                for i in range(2):
-                    words = xr[q][:, i, :].bitcast(F32)
-                    for u in range(2):
-                        nc.tensor.transpose(tp[:, u, 128 * i:128 * i + 128],
-                                            words[:, 256 * g + u:256 * g + 256:2], ident[:])
-                dst = words_out[:, 512 * h:512 * h + 512].rearrange("p (r u) -> p r u", u=2)
-                nc.scalar.copy(out=dst, in_=tp[:].rearrange("p u r -> p r u"))
-            nc.vector.quantize_mx(out=xc[b][:, gs[0]:gs[-1] + 1, :].rearrange("p g n -> p (g n)").bitcast(FP8X4),
-                                  scales=xs[b][:, gs[0]:gs[-1] + 1, :].rearrange("p g n -> p (g n)"), in_=t[:])
+        xr, ob, w1r, w2r, wi, xi, tps, accs, hp, hi, ps, ep = {}, {}, {}, {}, {}, {}, {}, {}, {}, {}, {}, {}
+        copy = {True: nc.vector.tensor_copy, False: nc.scalar.copy}
 
-        def mm1(acc, b, half, t, g):
-            c0 = 512 * half + 128 * t
-            n = 256 * len(class_blocks[b])
-            nc.tensor.matmul_mx(out=acc[:, :n],
-                                lhsT=w1c[:, g, c0:c0 + 128].bitcast(FP8X4),
-                                lhsT_scale=w1s[:, g, c0:c0 + 128],
-                                rhs=xc[b][:, g, :].bitcast(FP8X4),
-                                rhs_scale=xs[b][:, g, :],
-                                start=(g == 0), stop=(g == G1 - 1))
-
-        def new_accs():
-            return [psum.tile([P, 512], F32, name="acc") for t in range(4)]
-
-        def relu(acc, b, half, t):
-            n = 256 * len(class_blocks[b])
-            if t == 0:
-                hp[b, half] = hid.tile([P, 4, 512], BF16, name="hp")
-            nc.scalar.activation(hp[b, half][:, t, :n], acc[:, :n], ACT.Relu, bias=b1c[:, half, t:t + 1])
-
-        def h_prep(b, half, engine):
-            n = 256 * len(class_blocks[b])
-            t = inter.tile([P, 2048], BF16, name="il", align_bytes=64)
-            engine(out=t[:, :4 * n].rearrange("p (c i t) -> p c t i", i=4, t=4),
-                   in_=hp[b, half][:, :, :n].rearrange("p t (c i) -> p c t i", i=4))
-            nc.vector.quantize_mx(out=hc[b][:, half, :].bitcast(FP8X4), scales=hs[b][:, half, :], in_=t[:, :4 * n])
-
-        w2r = {}
+        def load_w1(half, g):
+            w1r[half, g] = raw.tile([P, 4, 512], BF16, name="wraw")
+            nc.sync.dma_start(out=w1r[half, g][:], in_=w1_v[g][:, :, 512 * half:512 * half + 512])
 
         def load_w2(g):
             for c0, c1 in ((0, 512), (512, 768)):
-                t = raw.tile([P, 4, c1 - c0], BF16, name="w1r")
-                nc.sync.dma_start(out=t[:], in_=w2_v[g][:, :, c0:c1])
-                w2r[g, c0] = t
+                w2r[g, c0] = raw.tile([P, 4, c1 - c0], BF16, name="wraw")
+                nc.sync.dma_start(out=w2r[g, c0][:], in_=w2_v[g][:, :, c0:c1])
 
-        def w2_prep(g, engine):
-            for c0, c1 in ((0, 512), (512, 768)):
-                t = inter.tile([P, 2048], BF16, name="il", align_bytes=64)
-                n = 4 * (c1 - c0)
-                engine(out=t[:, :n].rearrange("p (c i j) -> p c j i", i=4, j=4),
-                       in_=w2r[g, c0][:].rearrange("p j (c i) -> p c j i", i=4))
-                nc.vector.quantize_mx(out=w2c[:, g, c0:c1].bitcast(FP8X4), scales=w2s[:, g, c0:c1], in_=t[:, :n])
+        def row_tile(q, g):
+            if (q, g) not in xr:
+                xr[q, g] = rows.tile([P, 2, 512], BF16, name="xr%d" % g, align_bytes=64)
+            return xr[q, g]
 
-        def stage2(b, q, split):
-            h = class_blocks[b].index(q)
-            mean_sb = outp.tile([P, 2, L], F32, name="mean_sb")
-            std_sb = outp.tile([P, 2, L], F32, name="std_sb")
-            smp = outp.tile([P, 2, L], F32, name="smp")
+        def load_state(q, g):
+            nc.sync.dma_start(out=row_tile(q, g)[:], in_=state_v[:, 2 * q:2 * q + 2, 512 * g:512 * g + 512])
 
-            def sample(s):
-                nc.scalar.activation(smp[:, s, :], std_sb[:, s, :], ACT.Sqrt)
-                nc.vector.tensor_mul(out=smp[:, s, :], in0=smp[:, s, :], in1=eps_sb[:, 2 * q + s.start:2 * q + s.stop, :])
-                nc.vector.tensor_add(out=smp[:, s, :], in0=smp[:, s, :], in1=mean_sb[:, s, :])
+        def load_obs(q):
+            ob[q] = keep.tile([P, 2, O], U8, name="ob%d" % q)
+            nc.sync.dma_start(out=ob[q][:], in_=bytes_v[:, 2 * q:2 * q + 2, :])
 
+        def load_action(q):
+            nc.sync.dma_start(out=row_tile(q, 2)[:, :, :A], in_=action_v[:, 2 * q:2 * q + 2, :])
+
+        def product(q, g):
+            k0 = max(512 * g, S + A)
+            c0, c1 = k0 - (S + A), 512 * g + 512 - (S + A)
             for i in range(2):
-                r0 = 256 * h + 128 * i
-                for part in (1, 0):
-                    ps = psum.tile([P, 512], F32, name="tp")
-                    for c0, c1 in ((0, 256), (256, 384)):
-                        w0, w1_ = L * part + c0, L * part + c1
-                        for g in range(G2):
-                            nc.tensor.matmul_mx(out=ps[:, c0:c1],
-                                                lhsT=hc[b][:, g, r0:r0 + 128].bitcast(FP8X4),
-                                                lhsT_scale=hs[b][:, g, r0:r0 + 128],
-                                                rhs=w2c[:, g, w0:w1_].bitcast(FP8X4),
-                                                rhs_scale=w2s[:, g, w0:w1_],
-                                                start=(g == 0), stop=(g == G2 - 1))
-                    dst = std_sb if part else mean_sb
-                    nc.vector.tensor_add(out=dst[:, i, :], in0=ps[:, :L], in1=b2b[:, L * part:L * part + L])
-                if split:
-                    sample(slice(i, i + 1))
-            if not split:
-                sample(slice(0, 2))
-            nc.sync.dma_start(out=std_v[:, 2 * q:2 * q + 2, :], in_=std_sb[:])
-            nc.sync.dma_start(out=mean_v[:, 2 * q:2 * q + 2, :], in_=mean_sb[:])
-            nc.sync.dma_start(out=sample_v[:, 2 * q:2 * q + 2, :], in_=smp[:])
+                nc.vector.tensor_tensor(out=row_tile(q, g)[:, i, k0 - 512 * g:],
+                                        in0=ob[q][:, i, c0:c1].bitcast(FP8),
+                                        in1=scale[:, c0:c1], op=ALU.mult)
+
+        def turn(q, g):
+            tp = psum.tile([P, 2, 256], F32, name="tp")
+            for i in range(2):
+                words = xr[q, g][:, i, :].bitcast(F32)
+                for u in range(2):
+                    nc.tensor.transpose(tp[:, u, P * i:P * i + P], words[:, u::2], ident[:])
+            tps[q, g] = tp
+
+        def woven_tile(on_vector):
+            return inter.tile([P, 2048], BF16, name="woven_v" if on_vector else "woven_s", align_bytes=64, bufs=2 if on_vector else 3)
+
+        def drain(units):
+            t = woven_tile(False)
+            for h, (q, g) in enumerate(units):
+                nc.scalar.copy(out=t[:].bitcast(F32)[:, 512 * h:512 * h + 512].rearrange("p (r u) -> p r u", u=2),
+                               in_=tps[q, g][:].rearrange("p u r -> p r u"))
+            xi[units[0]] = t
+
+        def quant_x(b, g0, g1):
+            nc.vector.quantize_mx(out=xc[b][:, g0:g1, :].rearrange("p g n -> p (g n)").bitcast(FP8X4),
+                                  scales=xs[b][:, g0:g1, :].rearrange("p g n -> p (g n)"),
+                                  in_=xi[blocks[b][0], g0][:])
+
+        def weave_w1(half, g, on_vector):
+            if (half, g) not in wi:
+                wi[half, g] = inter.tile([P, 2048], BF16, name="woven_w", align_bytes=64)
+            cut = share(half, g)
+            part = slice(0, cut) if on_vector else slice(cut, 64)
+            copy[on_vector](out=wi[half, g][:].rearrange("p (t m e j) -> p m j e t", t=4, e=2, j=4)[:, part],
+                            in_=w1r[half, g][:].rearrange("p j (m e t) -> p m j e t", e=2, t=4)[:, part])
+
+        def share(half, g):
+            return 64 if (half, g) == (0, 0) else SHARE[half]
+
+        def quant_w1(half, g):
+            cols = slice(512 * half, 512 * half + 512)
+            nc.vector.quantize_mx(out=w1c[:, g, cols].bitcast(FP8X4), scales=w1s[:, g, cols], in_=wi[half, g][:])
+
+        def weave(dst, src, on_vector):
+            copy[on_vector](out=dst.rearrange("p (c i j) -> p c j i", i=8, j=4),
+                            in_=src.rearrange("p j (c i) -> p c j i", i=8))
+
+        def weave_w2(g, c0, on_vector):
+            t = woven_tile(on_vector)
+            n = w2r[g, c0].shape[2]
+            weave(t[:, :4 * n], w2r[g, c0][:], on_vector)
+            wi[2, g, c0] = t
+
+        def quant_w2(g, c0):
+            n = w2r[g, c0].shape[2]
+            nc.vector.quantize_mx(out=w2c[:, g, c0:c0 + n].bitcast(FP8X4), scales=w2s[:, g, c0:c0 + n],
+                                  in_=wi[2, g, c0][:, :4 * n])
+
+        def mm1(out, b, half, t, g):
+            cols = slice(512 * half + P * t, 512 * half + P * t + P)
+            xb, r0, n = spans[b]
+            nc.tensor.matmul_mx(out=out, lhsT=w1c[:, g, cols].bitcast(FP8X4), lhsT_scale=w1s[:, g, cols],
+                                rhs=xc[xb][:, g, r0:r0 + n].bitcast(FP8X4), rhs_scale=xs[xb][:, g, r0:r0 + n],
+                                start=(g == 0), stop=(g == G1 - 1))
+
+        def hidden_pass(b, half, g):
+            for t in range(4):
+                if g == 0:
+                    acc = psum.tile([P, 512], F32, name="acc")
+                    accs[b, half, t] = acc[:, :256 * len(blocks[b])]
+                mm1(accs[b, half, t], b, half, t, g)
+
+        def hidden_pair(b, half, t0, tag):
+            n = spans[b][2]
+            acc = psum.tile([P, 512 // n, n], F32, name=tag)
+            for t in range(t0, t0 + 512 // n):
+                accs[b, half, t] = acc[:, t - t0, :]
+                for g in range(G1):
+                    mm1(accs[b, half, t], b, half, t, g)
+
+        def relu(b, half, t):
+            n = spans[b][2]
+            if t == 0:
+                hp[b, half] = hid.tile([P, 4, n], BF16, name="hp%d" % n)
+            nc.scalar.activation(hp[b, half][:, t, :n], accs[b, half, t], ACT.Relu, bias=b1c[:, half, t:t + 1])
+
+        def weave_h(b, half, on_vector):
+            n = spans[b][2]
+            t = woven_tile(on_vector)
+            weave(t[:, :4 * n], hp[b, half][:, :, :n], on_vector)
+            hi[b, half] = t[:, :4 * n]
+
+        def quant_h(b, half):
+            nc.vector.quantize_mx(out=hc[b][:, half, :].bitcast(FP8X4), scales=hs[b][:, half, :], in_=hi[b, half])
+
+        def mm2(out, n, c0, c1):
+            b = span_of[n]
+            r0 = P * (n - first_tile[b])
+            for g in range(G2):
+                nc.tensor.matmul_mx(out=out, lhsT=hc[b][:, g, r0:r0 + P].bitcast(FP8X4),
+                                    lhsT_scale=hs[b][:, g, r0:r0 + P],
+                                    rhs=w2c[:, g, c0:c1].bitcast(FP8X4), rhs_scale=w2s[:, g, c0:c1],
+                                    start=(g == 0), stop=(g == G2 - 1))
+
+        def heads(n):
+            for c0, c1 in ((256, 2 * L), (0, 256)):
+                ps[n, c0] = psum.tile([P, c1 - c0], F32, name="tp")
+                mm2(ps[n, c0][:], n, c0, c1)
+
+        def bias_wide(n):
+            res = outp.tile([P, 2 * L], F32, name="res")
+            smp = outp.tile([P, L], F32, name="smp")
+            ep[n] = (res, smp)
+            nc.vector.tensor_add(out=res[:, 256:], in0=ps[n, 256][:], in1=b2b[:, 256:])
+
+        def bias_narrow(n):
+            nc.vector.tensor_add(out=ep[n][0][:, :256], in0=ps[n, 0][:], in1=b2b[:, :256])
+
+        def root(n):
+            nc.scalar.activation(ep[n][1][:], ep[n][0][:, L:], ACT.Sqrt)
+
+        def noise(n):
+            nc.vector.tensor_mul(out=ep[n][1][:], in0=ep[n][1][:], in1=eps_sb[:, n, :])
+
+        def shift(n):
+            nc.vector.tensor_add(out=ep[n][1][:], in0=ep[n][1][:], in1=ep[n][0][:, :L])
+
+        def store_std(n):
+            nc.sync.dma_start(out=std_v[:, n, :], in_=ep[n][0][:, L:])
+
+        def store_mean(n):
+            nc.sync.dma_start(out=mean_v[:, n, :], in_=ep[n][0][:, :L])
+
+        def store_sample(n):
+            nc.sync.dma_start(out=sample_v[:, n, :], in_=ep[n][1][:])
 
         srow = keep.tile([P, P], F32)
         nc.gpsimd.memset(srow[:], 0.0)
-        nc.sync.dma_start(out=srow[:15, :], in_=obs_scale.rearrange("o (c k) -> (o c) k", k=P))
-        scol = keep.tile([P, 16], F32)
-        tp = psum.tile([P, 512], F32, name="tp")
-        nc.tensor.transpose(tp[:, :P], srow[:], ident[:])
-        nc.scalar.copy(out=scol[:], in_=tp[:, :16])
-        for c0 in range(0, 15, 4):
-            c1 = min(c0 + 4, 15)
-            tp = psum.tile([P, 512], F32, name="tp")
-            for c in range(c0, c1):
-                nc.tensor.transpose(tp[:, P * (c - c0):P * (c - c0 + 1)], scol[:, c:c + 1].to_broadcast([P, P]), ident[:])
-            copy = nc.vector.tensor_copy if "SVSS"[c0 // 4] == "V" else nc.scalar.copy
-            copy(out=scale[:, P * c0:P * c1], in_=tp[:, :P * (c1 - c0)])
+        ident = keep.tile([P, P], F32)
+        make_identity(nc, ident[:])
+        warm = keep.tile([P, 1], F32)
+        nc.vector.memset(warm[:], 1.0)
+        nc.scalar.activation(warm[:], warm[:], ACT.Sqrt)
 
-        new_rows(0)
-        new_rows(1)
-        load_w1(0, 0)
-        load_obs(0)
-        load_state(0, 0, 1)
-        load_state(1, 0, 1)
-        load_w1(0, 1)
-        load_obs(1)
-        load_state(0, 1, 2)
-        load_state(1, 1, 2)
-        for g in range(2, 6):
-            load_w1(0, g)
-        nc.sync.dma_start(out=b1c[:], in_=b1.rearrange("(g p t) -> p g t", p=P, t=4))
-        load_w1(1, 0)
+        scol = keep.tile([P, SCALE_ROWS], F32)
 
-        load_w1(1, 1)
-        new_rows(2)
-        load_obs(2)
-        load_state(2, 0, 2)
-        load_w1(1, 2)
-        load_w1(1, 3)
-        new_rows(3)
-        load_obs(3)
-        load_state(3, 0, 2)
-        load_w1(1, 4)
-        load_w1(1, 5)
-        load_w2(0)
-        load_w2(1)
-        nc.sync.dma_start(out=b2b[:], in_=b2.partition_broadcast(P))
-        nc.sync.dma_start(out=eps_sb[:], in_=eps_v)
+        def load_scale():
+            nc.sync.dma_start(out=srow[:SCALE_ROWS, :SCALE_COLS],
+                              in_=obs_scale.rearrange("o (c k) -> (o c) k", k=SCALE_COLS))
 
-        vec, sca = nc.vector.tensor_copy, nc.scalar.copy
-        units = [(0, [g]) for g in range(6)] + [(1, [0, 1]), (1, [2, 3]), (1, [4, 5]), (2, [0, 1]), (2, [2, 3]), (2, [4, 5])]
-        tps, wi, xi, accs, hi, w2i, ps, ep = {}, {}, {}, {}, {}, {}, {}, {}
-        ENG = {"V": vec, "S": sca}
+        def load_b1():
+            nc.sync.dma_start(out=b1c[:], in_=b1.rearrange("(g p t) -> p g t", p=P, t=4))
 
-        def il(n):
-            wi[n] = interleave_w1(n // 6, n % 6, ENG["VSSSSVSSVVSV"[n]])
+        def load_b2():
+            nc.sync.dma_start(out=b2b[:], in_=b2.partition_broadcast(P))
 
-        def wq(n):
-            quant_w1(n // 6, n % 6, wi[n])
+        def load_eps():
+            nc.sync.dma_start(out=eps_sb[:], in_=eps_v)
 
-        def T(u):
-            b, gs = units[u]
-            tps[u] = []
-            for g in gs:
-                for q in class_blocks[b]:
-                    tp = psum.tile([P, 2, 256], F32, name="tp")
-                    for i in range(2):
-                        words = xr[q][:, i, :].bitcast(F32)
-                        for w in range(2):
-                            nc.tensor.transpose(tp[:, w, 128 * i:128 * i + 128],
-                                                words[:, 256 * g + w:256 * g + 256:2], ident[:])
-                    tps[u].append(tp)
+        def turn_scale():
+            tps["scale"] = psum.tile([P, 512], F32, name="tp")
+            nc.tensor.transpose(tps["scale"][:, :P], srow[:], ident[:])
 
-        def Cx(u):
-            t = inter.tile([P, 2048], BF16, name="il", align_bytes=64)
-            for h, tp in enumerate(tps[u]):
-                nc.scalar.copy(out=t[:].bitcast(F32)[:, 512 * h:512 * h + 512].rearrange("p (r u) -> p r u", u=2),
-                               in_=tp[:].rearrange("p u r -> p r u"))
-            xi[u] = t
+        def drain_scale():
+            nc.scalar.copy(out=scol[:], in_=tps["scale"][:, :SCALE_ROWS])
 
-        def Q(u):
-            b, gs = units[u]
-            nc.vector.quantize_mx(out=xc[b][:, gs[0]:gs[-1] + 1, :].rearrange("p g n -> p (g n)").bitcast(FP8X4),
-                                  scales=xs[b][:, gs[0]:gs[-1] + 1, :].rearrange("p g n -> p (g n)"), in_=xi[u][:])
+        def spread_scale(n):
+            tps["scale", n] = psum.tile([P, 4, P], F32, name="acc")
+            for c in range(4):
+                nc.tensor.transpose(tps["scale", n][:, c, :], scol[:, 4 * n + c:4 * n + c + 1].to_broadcast([P, P]), ident[:])
 
-        def PR(k):
-            if k < 8:
-                product((k // 2) % 2, k % 2, 0 if k < 4 else 896, 896 if k < 4 else O)
+        def drain_spread(n):
+            nc.scalar.copy(out=scale[:, 4 * SCALE_COLS * n:4 * SCALE_COLS * (n + 1)].rearrange("p (c k) -> p c k", c=4),
+                           in_=tps["scale", n][:, :, :SCALE_COLS])
+
+        def relus(b, half, t0):
+            relu(b, half, t0)
+            relu(b, half, t0 + 1)
+
+        def drain_x(b, n):
+            drain([(0, n), (1, n)] if b == 0 else [(b + 1, 2 * n), (b + 1, 2 * n + 1)])
+
+        def quant_xn(b, n):
+            if b == 0:
+                quant_x(0, n, n + 1)
             else:
-                product(2 + (k - 8) // 2, k % 2, 0, O)
+                quant_x(b, 2 * n, 2 * n + 2)
 
-        def M(b, half, g):
-            if g == 0:
-                accs[b, half] = new_accs()
-            for tt in range(4):
-                mm1(accs[b, half][tt], b, half, tt, g)
+        def weave_w1n(half, g):
+            weave_w1(half, g, True)
 
-        def R(b, half):
-            for tt in range(4):
-                relu(accs[b, half][tt], b, half, tt)
+        def weave_w1s(half, g):
+            weave_w1(half, g, False)
 
-        def C1(b, half, tt):
-            acc = psum.tile([P, 512], F32, name="acc")
-            for g in range(G1):
-                mm1(acc, b, half, tt, g)
-            accs[b, half, tt] = acc
+        w2_parts = [(g, c0) for g in range(G2) for c0 in (0, 512)]
 
-        def R1(b, half, tt):
-            relu(accs[b, half, tt], b, half, tt)
+        def weave_w2n(n):
+            weave_w2(w2_parts[n][0], w2_parts[n][1], n in W2V)
 
-        def HI(b, half):
-            n = 256 * len(class_blocks[b])
-            t = inter.tile([P, 2048], BF16, name="il", align_bytes=64)
-            ENG[["SS","SS","SS"][b][half]](
-                out=t[:, :4 * n].rearrange("p (c i t) -> p c t i", i=4, t=4),
-                in_=hp[b, half][:, :, :n].rearrange("p t (c i) -> p c t i", i=4))
-            hi[b, half] = t
+        def quant_w2n(n):
+            quant_w2(w2_parts[n][0], w2_parts[n][1])
 
-        def HQ(b, half):
-            n = 256 * len(class_blocks[b])
-            nc.vector.quantize_mx(out=hc[b][:, half, :].bitcast(FP8X4), scales=hs[b][:, half, :], in_=hi[b, half][:, :4 * n])
+        def weave_hn(b, half):
+            weave_h(b, half, (b, half) in HV)
 
-        def W2RANGE(k):
-            return k // 2, 512 * (k % 2), 512 + 256 * (k % 2)
+        def pair(b, half, t0):
+            hidden_pair(b, half, t0, "tp" if (b, half) == (1, 0) else "acc")
 
-        def WI(k):
-            g, c0, c1 = W2RANGE(k)
-            t = inter.tile([P, 2048], BF16, name="il", align_bytes=64)
-            ENG["VVVS"[k]](out=t[:, :4 * (c1 - c0)].rearrange("p (c i j) -> p c j i", i=4, j=4),
-                               in_=w2r[g, c0][:].rearrange("p j (c i) -> p c j i", i=4))
-            w2i[k] = t
+        block_of = [0, 0, 1, 2]
+        units = [G1, G1 // 2, G1 // 2]
 
-        def WQ(k):
-            g, c0, c1 = W2RANGE(k)
-            nc.vector.quantize_mx(out=w2c[:, g, c0:c1].bitcast(FP8X4), scales=w2s[:, g, c0:c1], in_=w2i[k][:, :4 * (c1 - c0)])
+        def needs(step):
+            f, a = step[0], step[1:]
+            if f == turn_scale:
+                return [(load_scale,)]
+            if f == drain_scale:
+                return [(turn_scale,)]
+            if f == spread_scale:
+                return [(drain_scale,)]
+            if f == drain_spread:
+                return [(spread_scale, a[0])]
+            if f == product:
+                return [(load_obs, a[0])] + [(drain_spread, n) for n in range(a[1] - 1)]
+            if f == turn:
+                return [(load_state, a[0], a[1])] if a[1] < 2 else [(product, a[0], a[1])] + [(load_action, a[0])]
+            if f == drain_x:
+                return [(turn, 0, a[1]), (turn, 1, a[1])] if a[0] == 0 else [(turn, a[0] + 1, 2 * a[1]), (turn, a[0] + 1, 2 * a[1] + 1)]
+            if f == quant_xn:
+                return [(drain_x,) + a]
+            if f in (weave_w1n, weave_w1s):
+                return [(load_w1,) + a]
+            if f == quant_w1:
+                return [(weave_w1n,) + a] + ([(weave_w1s,) + a] if share(*a) < 64 else [])
+            if f == weave_w2n:
+                return [(load_w2, a[0] // 2)]
+            if f == quant_w2n:
+                return [(weave_w2n,) + a]
+            if f == hidden_pass:
+                return [(quant_w1, a[1], a[2]), (quant_xn, 0, a[2])] + ([(hidden_pass, 0, a[1], a[2] - 1)] if a[2] else [])
+            if f == pair:
+                return [(quant_w1, a[1], g) for g in range(G1)] + [(quant_xn, spans[a[0]][0], n) for n in range(3)]
+            if f == relus:
+                return [(load_b1,), (hidden_pass, 0, a[1], G1 - 1) if a[0] == 0 else (pair, a[0], a[1], a[2] if a[0] == 1 else 0)] + ([(relus, a[0], a[1], 0)] if a[2] else [])
+            if f == weave_hn:
+                return [(relus, a[0], a[1], 0), (relus, a[0], a[1], 2)]
+            if f == quant_h:
+                return [(weave_hn,) + a]
+            if f == heads:
+                return [(quant_h, span_of[a[0]], 0), (quant_h, span_of[a[0]], 1)] + [(quant_w2n, n) for n in range(4)]
+            if f == bias_wide:
+                return [(heads, a[0]), (load_b2,)]
+            if f in (bias_narrow, root, store_std):
+                return [(bias_wide,) + a]
+            if f == noise:
+                return [(root,) + a, (load_eps,)]
+            if f == shift:
+                return [(noise,) + a, (bias_narrow, a[0])]
+            if f == store_mean:
+                return [(bias_narrow,) + a]
+            if f == store_sample:
+                return [(shift,) + a]
+            return []
 
-        def S2(q, i):
-            b = 0 if q < 2 else q - 1
-            r0 = 256 * class_blocks[b].index(q) + 128 * i
-            for part in (1, 0):
-                acc = psum.tile([P, 512], F32, name="tp")
-                for c0, c1 in ((0, 256), (256, 384)):
-                    w0, w9 = L * part + c0, L * part + c1
-                    for g in range(G2):
-                        nc.tensor.matmul_mx(out=acc[:, c0:c1],
-                                            lhsT=hc[b][:, g, r0:r0 + 128].bitcast(FP8X4),
-                                            lhsT_scale=hs[b][:, g, r0:r0 + 128],
-                                            rhs=w2c[:, g, w0:w9].bitcast(FP8X4),
-                                            rhs_scale=w2s[:, g, w0:w9],
-                                            start=(g == 0), stop=(g == G2 - 1))
-                ps[q, i, part] = acc
+        def takes(step):
+            f, a = step[0], step[1:]
+            woven = {True: "woven_v", False: "woven_s"}
+            if f == load_w1:
+                return [("wraw", 7, [(weave_w1n,) + a] + ([(weave_w1s,) + a] if share(*a) < 64 else []))]
+            if f == load_w2:
+                return [("wraw", 7, [(weave_w2n, 2 * a[0] + n)]) for n in range(2)]
+            if f in (load_state, product) and (a[0], a[1]) not in xr:
+                return [("xr%d" % a[1], 3, [(turn,) + a])]
+            if f == load_action and (a[0], 2) not in xr:
+                return [("xr2", 3, [(turn, a[0], 2)])]
+            if f == drain_x:
+                return [("woven_s", 3, [(quant_xn,) + a])]
+            if f in (weave_w1n, weave_w1s) and a not in wi:
+                return [("woven_w", 3, [(quant_w1,) + a])]
+            if f == weave_w2n:
+                return [(woven[a[0] in W2V], 2 if a[0] in W2V else 3, [(quant_w2n,) + a])]
+            if f == weave_hn:
+                return [(woven[a in HV], 2 if a in HV else 3, [(quant_h,) + a])]
+            if f == turn_scale:
+                return [("tp", 4, [(drain_scale,)])]
+            if f == spread_scale:
+                return [("acc", 4, [(drain_spread,) + a])]
+            if f == turn:
+                return [("tp", 4, [(drain_x, block_of[a[0]], a[1] if a[0] < 2 else a[1] // 2)])]
+            if f == hidden_pass and a[2] == 0:
+                return [("acc", 4, [(relus, 0, a[1], 2 * (t // 2))]) for t in range(4)]
+            if f == pair:
+                return [("tp" if a[:2] == (1, 0) else "acc", 4, [(relus, a[0], a[1], a[2] if a[0] == 1 else 2)])]
+            if f == relus and a[2] == 0:
+                return [("hp%d" % spans[a[0]][2], 2, [(weave_hn, a[0], a[1])])]
+            if f == heads:
+                return [("tp", 4, [(bias_wide, a[0])]), ("tp", 4, [(bias_narrow, a[0])])]
+            if f == bias_wide:
+                return [("res", 4, [(store_std,) + a, (store_mean,) + a, (store_sample,) + a])]
+            return []
 
-        def BA(q, i):
-            if q not in ep:
-                mean_sb = outp.tile([P, 2, L], F32, name="mean_sb")
-                std_sb = outp.tile([P, 2, L], F32, name="std_sb")
-                smp = outp.tile([P, 2, L], F32, name="smp")
-                ep[q] = (mean_sb, std_sb, smp)
-            for part in (1, 0):
-                nc.vector.tensor_add(out=ep[q][part][:, i, :], in0=ps[q, i, part][:, :L], in1=b2b[:, L * part:L * part + L])
+        def rows_of(q):
+            return [(load_obs, q), (load_state, q, 0), (load_state, q, 1), (load_action, q)]
 
-        def SQ(q, i):
-            nc.scalar.activation(ep[q][2][:, i[0]:i[-1] + 1, :], ep[q][1][:, i[0]:i[-1] + 1, :], ACT.Sqrt)
+        def pair_of_turns(n):
+            return [(turn, 0, n), (turn, 1, n)] if n < G1 else [(turn, n // 3, 2 * (n % 3)), (turn, n // 3, 2 * (n % 3) + 1)]
 
-        def MU(q, i):
-            s = ep[q][2][:, i[0]:i[-1] + 1, :]
-            nc.vector.tensor_mul(out=s, in0=s, in1=eps_sb[:, 2 * q + i[0]:2 * q + i[-1] + 1, :])
+        def both_relus(b, half):
+            return [(relus, b, half, 0), (relus, b, half, 2)]
 
-        def AD(q, i):
-            s = ep[q][2][:, i[0]:i[-1] + 1, :]
-            nc.vector.tensor_add(out=s, in0=s, in1=ep[q][0][:, i[0]:i[-1] + 1, :])
+        small = [(2, 0), (2, 1), (3, 0), (3, 1)]
 
-        def OUT(q):
-            for view, part in ((std_v, 1), (mean_v, 0), (sample_v, 2)):
-                nc.sync.dma_start(out=view[:, 2 * q:2 * q + 2, :], in_=ep[q][part][:])
+        sync_q = [(load_scale,), (load_w1, 0, 0), (load_obs, 0), (load_state, 0, 0), (load_state, 1, 0), (load_w1, 0, 1),
+                  (load_obs, 1), (load_state, 0, 1), (load_state, 1, 1), (load_action, 0), (load_action, 1)]
+        sync_q += [(load_w1, 0, g) for g in range(2, G1)] + [(load_b1,)] + rows_of(2)
+        sync_q += [(load_w1, 1, g) for g in range(G1)] + rows_of(3)
+        sync_q += [(load_w2, 0), (load_w2, 1), (load_b2,), (load_eps,)]
+        for n in range(NT):
+            sync_q += [(store_std, n), (store_mean, n)] + ([(store_sample, n - 1)] if n else [])
+        sync_q += [(store_sample, NT - 1)]
 
-        with tc.manual_schedule(engines={mybir.EngineType.PE, mybir.EngineType.DVE, mybir.EngineType.Activation}):
-            il(0)
-            T(0)
-            PR(5)
-            PR(0)
-            PR(4)
-            Cx(0)
-            Q(0)
-            PR(1)
-            PR(2)
-            il(1)
-            T(1)
-            wq(0)
-            Cx(1)
-            Q(1)
-            il(2)
-            PR(3)
-            PR(7)
-            wq(1)
-            il(3)
-            il(5)
-            T(2)
-            wq(2)
-            Cx(2)
-            wq(5)
-            T(3)
-            PR(6)
-            Cx(3)
-            il(7)
-            T(4)
-            T(5)
-            il(4)
-            Cx(4)
-            wq(3)
-            Cx(5)
-            PR(9)
-            Q(2)
-            M(0, 0, 0)
-            il(6)
-            PR(8)
-            Q(3)
-            wq(4)
-            M(0, 0, 1)
-            il(8)
-            M(0, 0, 2)
-            Q(4)
-            Q(5)
-            il(11)
-            T(6)
-            Cx(6)
-            wq(7)
-            T(8)
-            M(0, 0, 3)
-            M(0, 0, 4)
-            il(9)
-            wq(6)
-            Cx(8)
-            M(0, 0, 5)
-            wq(11)
-            wq(9)
-            T(9)
-            T(7)
-            R(0, 0)
-            il(10)
-            HI(0, 0)
-            wq(8)
-            M(0, 1, 0)
-            Cx(7)
-            M(0, 1, 1)
-            wq(10)
-            PR(11)
-            M(0, 1, 2)
-            PR(10)
-            M(0, 1, 3)
-            Q(7)
-            Q(6)
-            Q(8)
-            M(0, 1, 4)
-            Cx(9)
-            M(0, 1, 5)
-            T(10)
-            T(11)
-            WI(0)
-            R(0, 1)
-            Cx(11)
-            HQ(0, 0)
-            HI(0, 1)
-            M(1, 0, 0)
-            M(1, 0, 1)
-            M(1, 0, 2)
-            M(1, 0, 3)
-            M(1, 0, 4)
-            WI(1)
-            WI(2)
-            WQ(0)
-            M(1, 0, 5)
-            R(1, 0)
-            HQ(0, 1)
-            C1(1, 1, 3)
-            WI(3)
-            WQ(1)
-            C1(1, 1, 0)
-            Cx(10)
-            R1(1, 1, 0)
-            C1(1, 1, 1)
-            WQ(2)
-            R1(1, 1, 1)
-            WQ(3)
-            C1(1, 1, 2)
-            S2(0, 1)
-            Q(9)
-            Q(11)
-            R1(1, 1, 2)
-            S2(0, 0)
-            BA(0, 1)
-            R1(1, 1, 3)
-            Q(10)
-            HI(1, 0)
-            BA(0, 0)
-            M(2, 0, 0)
-            S2(1, 0)
-            M(2, 0, 1)
-            SQ(0, (0,1))
-            BA(1, 0)
-            M(2, 0, 2)
-            HI(1, 1)
-            MU(0, (0,1))
-            AD(0, (0,1))
-            M(2, 0, 3)
-            M(2, 0, 4)
-            M(2, 0, 5)
-            S2(1, 1)
-            R(2, 0)
-            BA(1, 1)
-            C1(2, 1, 0)
-            OUT(0)
-            C1(2, 1, 1)
-            C1(2, 1, 2)
-            HQ(1, 1)
-            HQ(1, 0)
-            SQ(1, (0,1))
-            C1(2, 1, 3)
-            S2(2, 1)
-            MU(1, (0,1))
-            R1(2, 1, 0)
-            AD(1, (0,1))
-            OUT(1)
-            R1(2, 1, 1)
-            HI(2, 0)
-            HQ(2, 0)
-            BA(2, 1)
-            R1(2, 1, 2)
-            S2(2, 0)
-            R1(2, 1, 3)
-            BA(2, 0)
-            HI(2, 1)
-            SQ(2, (0,1))
-            HQ(2, 1)
-            S2(3, 1)
-            MU(2, (0,1))
-            BA(3, 1)
-            S2(3, 0)
-            BA(3, 0)
-            AD(2, (0,1))
-            OUT(2)
-            SQ(3, (0,))
-            MU(3, (0,))
-            SQ(3, (1,))
-            MU(3, (1,))
-            AD(3, (0,))
-            AD(3, (1,))
-            OUT(3)
+        tensor_q = [(turn_scale,)] + [(spread_scale, n) for n in range(4)]
+        for n in range(LEAD):
+            tensor_q += pair_of_turns(n)
+        for g in range(G1):
+            tensor_q += [(hidden_pass, 0, 0, g)] + pair_of_turns(g + LEAD)
+        tensor_q += [(hidden_pass, 0, 1, 0), (pair, 1, 0, 0), (pair, 1, 0, 2)]
+        tensor_q += [(hidden_pass, 0, 1, g) for g in range(1, G1)]
+        tensor_q += pair_of_turns(9) + [(pair, 1, 1, 0)] + pair_of_turns(10) + [(pair, 1, 1, 2)] + pair_of_turns(11)
+        tensor_q += [(heads, 0), (heads, 1)]
+        for n, (b, half) in enumerate(small):
+            tensor_q += [(heads, n + 2), (pair, b, half, 0)]
+        tensor_q += [(heads, 6), (heads, 7)]
+
+        scalar_q = [(drain_scale,)] + [(drain_spread, n) for n in range(4)] + [(drain_x, 0, 0)]
+        for g in range(1, G1):
+            scalar_q += [(weave_w1s, 0, g), (drain_x, 0, g)]
+        scalar_q += [(drain_x, 1, 0), (weave_w1s, 1, 0), (drain_x, 1, 1)] + both_relus(0, 0) + [(drain_x, 1, 2)]
+        scalar_q += [(weave_w1s, 1, g) for g in range(1, G1)] + both_relus(1, 0) + [(weave_w2n, 0)]
+        scalar_q += both_relus(0, 1) + [(weave_hn, 0, 1)] + [(drain_x, 2, n) for n in range(3)] + both_relus(1, 1)
+        scalar_q += [(root, 0), (weave_hn, 1, 0), (root, 1), (weave_hn, 1, 1), (root, 2)]
+        for n, (b, half) in enumerate(small):
+            scalar_q += both_relus(b, half) + ([(weave_hn, b, half)] if (b, half) not in HV else []) + [(root, n + 3)]
+        scalar_q += [(root, 7)]
+
+        products = [(product, q, g) for g0 in (2, 4) for q, g in (((0, g0), (0, g0 + 1), (1, g0), (1, g0 + 1)) if g0 == 2 else ((0, 4), (1, 4), (0, 5), (1, 5)))]
+        products += [(product, q, g) for q in (2, 3) for g in range(2, G1)]
+        vector_q = []
+        for g in range(G1):
+            vector_q += [(weave_w1n, 0, g), products.pop(0), (quant_w1, 0, g)] + ([products.pop(0)] if g < 4 else []) + [(quant_xn, 0, g)]
+        vector_q += [(weave_w1n, 1, 0), products.pop(0), (quant_w1, 1, 0), products.pop(0), (quant_xn, 1, 0)]
+        vector_q += [(weave_w1n, 1, 1), (quant_xn, 1, 1), (weave_w1n, 1, 2), (quant_xn, 1, 2)]
+        for g in range(1, 4):
+            vector_q += [(quant_w1, 1, g), (weave_w1n, 1, g + 2)]
+        vector_q += [(quant_w1, 1, 4), products.pop(0), (quant_w1, 1, 5), products.pop(0)]
+        vector_q += [(weave_hn, 0, 0), products.pop(0), (quant_h, 0, 0), products.pop(0)]
+        for n, m in ((2, 0), (1, 2), (3, 1)):
+            vector_q += [(weave_w2n, n), (quant_w2n, m)]
+        vector_q += [(quant_w2n, 3), (quant_h, 0, 1), (quant_xn, 2, 0), (quant_xn, 2, 1)]
+        between = [[(quant_xn, 2, 2)], [(quant_h, 1, 0)], [(quant_h, 1, 1)], [(quant_h, 2, 0)], [(quant_h, 2, 1)], [(quant_h, 3, 0), (weave_hn, 3, 1)]]
+        for n in range(NT + 1):
+            vector_q += [(bias_wide, n)] if n < NT else []
+            vector_q += [(quant_h, 3, 1)] if n == 6 else []
+            vector_q += [(noise, n - 1)] if n else []
+            vector_q += [(bias_narrow, n)] if n < NT else []
+            vector_q += [(shift, n - 1)] if n else []
+            vector_q += between[n] if n < len(between) else []
+        done = set()
+        held = {}
+        queues = [sync_q, tensor_q, scalar_q, vector_q]
+        while any(queues):
+            moved = False
+            for queue in queues:
+                if not queue or not all(n in done for n in needs(queue[0])):
+                    continue
+                slots = takes(queue[0])
+                count = {}
+                free = True
+                for tag, bufs, readers in slots:
+                    count[tag] = count.get(tag, 0) + 1
+                    n = len(held.get(tag, [])) + count[tag] - 1 - bufs
+                    free = free and (n < 0 or all(r in done for r in held[tag][n]))
+                if not free:
+                    continue
+                for tag, bufs, readers in slots:
+                    held.setdefault(tag, []).append(readers)
+                step = queue.pop(0)
+                step[0](*step[1:])
+                done.add(step)
+                moved = True
+            assert moved

@@ -17,39 +17,44 @@ ACT = mybir.ActivationFunctionType
 ALU = mybir.AluOpType
 
 P = 128
-G1 = K1 // 512
-G2 = H // 512
+KP = 4 * P
+G1 = K1 // KP
+G2 = H // KP
 NT = B // P
-NQ = NT // 2
+QT = 2 * P
+STATE_PASSES = S // KP
+WOVEN = 4 * KP
+
 SCALE_ROWS = 16
 SCALE_COLS = O // SCALE_ROWS
-SHARE = (18, 32)
+
+GROUPS = ((0, 1), (2,), (3,))
+FRONT, THIRD, LAST, LAST_A, LAST_B = (0, 0, 2 * QT), (1, 0, QT), (2, 0, QT), (2, 0, P), (2, P, P)
+SPLIT = 2 * L - KP
+W2_PIECES = tuple((g, c0, min(KP, 2 * L - c0)) for g in range(G2) for c0 in (0, KP))
+
+RUNS = KP // 8
+VECTOR_RUNS = (18, 32)
 LEAD = 3
-W2V = (1, 2, 3)
-HV = ((0, 0), (3, 1))
+DEPTH = {"wraw": 6, "woven_w": 3, "woven_v": 2, "woven_s": 4, "rows": 3, "res": 4, "acc": 4, "tp": 4}
+HIDDEN_DEPTH = {2 * QT: 2, QT: 3, P: 2}
 
 
 def tile_rssm_pa_kernel(tc, prev_state, prev_action, obs_bytes, obs_scale, eps,
                                        w1, b1, w2, b2, out_mean, out_std, out_sample):
     nc = tc.nc
 
-    state_v = prev_state.rearrange("(p i) k -> p i k", i=NT)
-    action_v = prev_action.rearrange("(p i) k -> p i k", i=NT)
-    bytes_v = obs_bytes.rearrange("(p i) k -> p i k", i=NT)
-    eps_v = eps.rearrange("(p i) n -> p i n", i=NT)
-    mean_v = out_mean.rearrange("(p i) n -> p i n", i=NT)
-    std_v = out_std.rearrange("(p i) n -> p i n", i=NT)
-    sample_v = out_sample.rearrange("(p i) n -> p i n", i=NT)
-    w1_v = w1.rearrange("(g p j) c -> g p j c", p=P, j=4)
-    w2_v = w2.rearrange("(g p j) c -> g p j c", p=P, j=4)
+    def by_tile(ap):
+        return ap.rearrange("(p n) c -> p n c", n=NT)
+
+    state_v, action_v, bytes_v, eps_v = by_tile(prev_state), by_tile(prev_action), by_tile(obs_bytes), by_tile(eps)
+    mean_v, std_v, sample_v = by_tile(out_mean), by_tile(out_std), by_tile(out_sample)
+    w1_v = w1.rearrange("(g p t) c -> g p t c", p=P, t=4)
+    w2_v = w2.rearrange("(g p t) c -> g p t c", p=P, t=4)
 
     with ExitStack() as ctx:
         keep = ctx.enter_context(tc.tile_pool(name="keep", bufs=1))
-        rows = ctx.enter_context(tc.tile_pool(name="rows", bufs=3))
-        raw = ctx.enter_context(tc.tile_pool(name="raw", bufs=7))
-        inter = ctx.enter_context(tc.tile_pool(name="inter", bufs=3))
-        hid = ctx.enter_context(tc.tile_pool(name="hid", bufs=2))
-        outp = ctx.enter_context(tc.tile_pool(name="outp", bufs=4))
+        stream = ctx.enter_context(tc.tile_pool(name="stream", bufs=1))
         psum = ctx.enter_context(tc.psum_pool(name="psum", bufs=4))
         ctx.enter_context(tc.manual_schedule())
 
@@ -57,440 +62,394 @@ def tile_rssm_pa_kernel(tc, prev_state, prev_action, obs_bytes, obs_scale, eps,
         w1s = keep.tile([P, G1, H], U8, align_bytes=64)
         w2c = keep.tile([P, G2, 2 * L], U32, align_bytes=64)
         w2s = keep.tile([P, G2, 2 * L], U8, align_bytes=64)
+        xc, xs, hc, hs = [], [], [], []
+        for grp, quarters in enumerate(GROUPS):
+            n = QT * len(quarters)
+            xc.append(keep.tile([P, G1, n], U32, name="xc%d" % grp, align_bytes=64))
+            xs.append(keep.tile([P, G1, n], U8, name="xs%d" % grp, align_bytes=64))
+            hc.append(keep.tile([P, G2, n], U32, name="hc%d" % grp, align_bytes=64))
+            hs.append(keep.tile([P, G2, n], U8, name="hs%d" % grp, align_bytes=64))
+        scale_rows = keep.tile([P, P], F32)
+        scale_cols = keep.tile([P, SCALE_ROWS], F32)
         scale = keep.tile([P, O], F32)
-        b1c = keep.tile([P, G2, 4], BF16)
-        b2b = keep.tile([P, 2 * L], BF16)
+        b1_cols = keep.tile([P, G2, 4], BF16)
+        b2_rows = keep.tile([P, 2 * L], BF16)
         eps_sb = keep.tile([P, NT, L], BF16)
-        blocks = [[0, 1], [2], [3]]
-        xc, xs, hc, hs = {}, {}, {}, {}
-        for b, qs in enumerate(blocks):
-            n = 256 * len(qs)
-            xc[b] = keep.tile([P, G1, n], U32, name="xc%d" % b, align_bytes=64)
-            xs[b] = keep.tile([P, G1, n], U8, name="xs%d" % b, align_bytes=64)
-        spans = [(0, 0, 512), (1, 0, 256), (2, 0, 128), (2, 128, 128)]
-        span_of = [0, 0, 0, 0, 1, 1, 2, 3]
-        first_tile = [0, 4, 6, 7]
-        for b, (xb, r0, n) in enumerate(spans):
-            hc[b] = keep.tile([P, G2, n], U32, name="hc%d" % b, align_bytes=64)
-            hs[b] = keep.tile([P, G2, n], U8, name="hs%d" % b, align_bytes=64)
-
-        xr, ob, w1r, w2r, wi, xi, tps, accs, hp, hi, ps, ep = {}, {}, {}, {}, {}, {}, {}, {}, {}, {}, {}, {}
-        copy = {True: nc.vector.tensor_copy, False: nc.scalar.copy}
-
-        def load_w1(half, g):
-            w1r[half, g] = raw.tile([P, 4, 512], BF16, name="wraw")
-            nc.sync.dma_start(out=w1r[half, g][:], in_=w1_v[g][:, :, 512 * half:512 * half + 512])
-
-        def load_w2(g):
-            for c0, c1 in ((0, 512), (512, 768)):
-                w2r[g, c0] = raw.tile([P, 4, c1 - c0], BF16, name="wraw")
-                nc.sync.dma_start(out=w2r[g, c0][:], in_=w2_v[g][:, :, c0:c1])
-
-        def row_tile(q, g):
-            if (q, g) not in xr:
-                xr[q, g] = rows.tile([P, 2, 512], BF16, name="xr%d" % g, align_bytes=64)
-            return xr[q, g]
-
-        def load_state(q, g):
-            nc.sync.dma_start(out=row_tile(q, g)[:], in_=state_v[:, 2 * q:2 * q + 2, 512 * g:512 * g + 512])
-
-        def load_obs(q):
-            ob[q] = keep.tile([P, 2, O], U8, name="ob%d" % q)
-            nc.sync.dma_start(out=ob[q][:], in_=bytes_v[:, 2 * q:2 * q + 2, :])
-
-        def load_action(q):
-            nc.sync.dma_start(out=row_tile(q, 2)[:, :, :A], in_=action_v[:, 2 * q:2 * q + 2, :])
-
-        def product(q, g):
-            k0 = max(512 * g, S + A)
-            c0, c1 = k0 - (S + A), 512 * g + 512 - (S + A)
-            for i in range(2):
-                nc.vector.tensor_tensor(out=row_tile(q, g)[:, i, k0 - 512 * g:],
-                                        in0=ob[q][:, i, c0:c1].bitcast(FP8),
-                                        in1=scale[:, c0:c1], op=ALU.mult)
-
-        def turn(q, g):
-            tp = psum.tile([P, 2, 256], F32, name="tp")
-            for i in range(2):
-                words = xr[q, g][:, i, :].bitcast(F32)
-                for u in range(2):
-                    nc.tensor.transpose(tp[:, u, P * i:P * i + P], words[:, u::2], ident[:])
-            tps[q, g] = tp
-
-        def woven_tile(on_vector):
-            return inter.tile([P, 2048], BF16, name="woven_v" if on_vector else "woven_s", align_bytes=64, bufs=2 if on_vector else 3)
-
-        def drain(units):
-            t = woven_tile(False)
-            for h, (q, g) in enumerate(units):
-                nc.scalar.copy(out=t[:].bitcast(F32)[:, 512 * h:512 * h + 512].rearrange("p (r u) -> p r u", u=2),
-                               in_=tps[q, g][:].rearrange("p u r -> p r u"))
-            xi[units[0]] = t
-
-        def quant_x(b, g0, g1):
-            nc.vector.quantize_mx(out=xc[b][:, g0:g1, :].rearrange("p g n -> p (g n)").bitcast(FP8X4),
-                                  scales=xs[b][:, g0:g1, :].rearrange("p g n -> p (g n)"),
-                                  in_=xi[blocks[b][0], g0][:])
-
-        def weave_w1(half, g, on_vector):
-            if (half, g) not in wi:
-                wi[half, g] = inter.tile([P, 2048], BF16, name="woven_w", align_bytes=64)
-            cut = share(half, g)
-            part = slice(0, cut) if on_vector else slice(cut, 64)
-            copy[on_vector](out=wi[half, g][:].rearrange("p (t m e j) -> p m j e t", t=4, e=2, j=4)[:, part],
-                            in_=w1r[half, g][:].rearrange("p j (m e t) -> p m j e t", e=2, t=4)[:, part])
-
-        def share(half, g):
-            return 64 if (half, g) == (0, 0) else SHARE[half]
-
-        def quant_w1(half, g):
-            cols = slice(512 * half, 512 * half + 512)
-            nc.vector.quantize_mx(out=w1c[:, g, cols].bitcast(FP8X4), scales=w1s[:, g, cols], in_=wi[half, g][:])
-
-        def weave(dst, src, on_vector):
-            copy[on_vector](out=dst.rearrange("p (c i j) -> p c j i", i=8, j=4),
-                            in_=src.rearrange("p j (c i) -> p c j i", i=8))
-
-        def weave_w2(g, c0, on_vector):
-            t = woven_tile(on_vector)
-            n = w2r[g, c0].shape[2]
-            weave(t[:, :4 * n], w2r[g, c0][:], on_vector)
-            wi[2, g, c0] = t
-
-        def quant_w2(g, c0):
-            n = w2r[g, c0].shape[2]
-            nc.vector.quantize_mx(out=w2c[:, g, c0:c0 + n].bitcast(FP8X4), scales=w2s[:, g, c0:c0 + n],
-                                  in_=wi[2, g, c0][:, :4 * n])
-
-        def mm1(out, b, half, t, g):
-            cols = slice(512 * half + P * t, 512 * half + P * t + P)
-            xb, r0, n = spans[b]
-            nc.tensor.matmul_mx(out=out, lhsT=w1c[:, g, cols].bitcast(FP8X4), lhsT_scale=w1s[:, g, cols],
-                                rhs=xc[xb][:, g, r0:r0 + n].bitcast(FP8X4), rhs_scale=xs[xb][:, g, r0:r0 + n],
-                                start=(g == 0), stop=(g == G1 - 1))
-
-        def hidden_pass(b, half, g):
-            for t in range(4):
-                if g == 0:
-                    acc = psum.tile([P, 512], F32, name="acc")
-                    accs[b, half, t] = acc[:, :256 * len(blocks[b])]
-                mm1(accs[b, half, t], b, half, t, g)
-
-        def hidden_pair(b, half, t0, tag):
-            n = spans[b][2]
-            acc = psum.tile([P, 512 // n, n], F32, name=tag)
-            for t in range(t0, t0 + 512 // n):
-                accs[b, half, t] = acc[:, t - t0, :]
-                for g in range(G1):
-                    mm1(accs[b, half, t], b, half, t, g)
-
-        def relu(b, half, t):
-            n = spans[b][2]
-            if t == 0:
-                hp[b, half] = hid.tile([P, 4, n], BF16, name="hp%d" % n)
-            nc.scalar.activation(hp[b, half][:, t, :n], accs[b, half, t], ACT.Relu, bias=b1c[:, half, t:t + 1])
-
-        def weave_h(b, half, on_vector):
-            n = spans[b][2]
-            t = woven_tile(on_vector)
-            weave(t[:, :4 * n], hp[b, half][:, :, :n], on_vector)
-            hi[b, half] = t[:, :4 * n]
-
-        def quant_h(b, half):
-            nc.vector.quantize_mx(out=hc[b][:, half, :].bitcast(FP8X4), scales=hs[b][:, half, :], in_=hi[b, half])
-
-        def mm2(out, n, c0, c1):
-            b = span_of[n]
-            r0 = P * (n - first_tile[b])
-            for g in range(G2):
-                nc.tensor.matmul_mx(out=out, lhsT=hc[b][:, g, r0:r0 + P].bitcast(FP8X4),
-                                    lhsT_scale=hs[b][:, g, r0:r0 + P],
-                                    rhs=w2c[:, g, c0:c1].bitcast(FP8X4), rhs_scale=w2s[:, g, c0:c1],
-                                    start=(g == 0), stop=(g == G2 - 1))
-
-        def heads(n):
-            for c0, c1 in ((256, 2 * L), (0, 256)):
-                ps[n, c0] = psum.tile([P, c1 - c0], F32, name="tp")
-                mm2(ps[n, c0][:], n, c0, c1)
-
-        def bias_wide(n):
-            res = outp.tile([P, 2 * L], F32, name="res")
-            smp = outp.tile([P, L], F32, name="smp")
-            ep[n] = (res, smp)
-            nc.vector.tensor_add(out=res[:, 256:], in0=ps[n, 256][:], in1=b2b[:, 256:])
-
-        def bias_narrow(n):
-            nc.vector.tensor_add(out=ep[n][0][:, :256], in0=ps[n, 0][:], in1=b2b[:, :256])
-
-        def root(n):
-            nc.scalar.activation(ep[n][1][:], ep[n][0][:, L:], ACT.Sqrt)
-
-        def noise(n):
-            nc.vector.tensor_mul(out=ep[n][1][:], in0=ep[n][1][:], in1=eps_sb[:, n, :])
-
-        def shift(n):
-            nc.vector.tensor_add(out=ep[n][1][:], in0=ep[n][1][:], in1=ep[n][0][:, :L])
-
-        def store_std(n):
-            nc.sync.dma_start(out=std_v[:, n, :], in_=ep[n][0][:, L:])
-
-        def store_mean(n):
-            nc.sync.dma_start(out=mean_v[:, n, :], in_=ep[n][0][:, :L])
-
-        def store_sample(n):
-            nc.sync.dma_start(out=sample_v[:, n, :], in_=ep[n][1][:])
-
-        srow = keep.tile([P, P], F32)
-        nc.gpsimd.memset(srow[:], 0.0)
         ident = keep.tile([P, P], F32)
-        make_identity(nc, ident[:])
         warm = keep.tile([P, 1], F32)
-        nc.vector.memset(warm[:], 1.0)
-        nc.scalar.activation(warm[:], warm[:], ACT.Sqrt)
 
-        scol = keep.tile([P, SCALE_ROWS], F32)
+        raw, woven, rows, obs, banks, hidden, result = {}, {}, {}, {}, {}, {}, {}
+        copy = {"vector": nc.vector.tensor_copy, "scalar": nc.scalar.copy}
+
+        def streamed(tag, shape, dtype):
+            return stream.tile(shape, dtype, name=tag, bufs=DEPTH[tag], align_bytes=64)
 
         def load_scale():
-            nc.sync.dma_start(out=srow[:SCALE_ROWS, :SCALE_COLS],
-                              in_=obs_scale.rearrange("o (c k) -> (o c) k", k=SCALE_COLS))
+            nc.sync.dma_start(out=scale_rows[:SCALE_ROWS, :SCALE_COLS],
+                              in_=obs_scale.rearrange("o (r c) -> (o r) c", c=SCALE_COLS))
+
+        def load_w1(half, g):
+            raw[half, g] = streamed("wraw", [P, 4, KP], BF16)
+            nc.sync.dma_start(out=raw[half, g][:], in_=w1_v[g][:, :, KP * half:KP * half + KP])
+
+        def load_w2(piece):
+            g, c0, n = piece
+            raw[piece] = streamed("wraw", [P, 4, n], BF16)
+            nc.sync.dma_start(out=raw[piece][:], in_=w2_v[g][:, :, c0:c0 + n])
+
+        def row_tile(q, g):
+            if (q, g) not in rows:
+                rows[q, g] = stream.tile([P, 2, KP], BF16, name="rows%d" % g, bufs=DEPTH["rows"], align_bytes=64)
+            return rows[q, g]
+
+        def load_state(q, g):
+            nc.sync.dma_start(out=row_tile(q, g)[:], in_=state_v[:, 2 * q:2 * q + 2, KP * g:KP * g + KP])
+
+        def load_action(q):
+            nc.sync.dma_start(out=row_tile(q, STATE_PASSES)[:, :, :A], in_=action_v[:, 2 * q:2 * q + 2, :])
+
+        def load_obs(q):
+            obs[q] = keep.tile([P, 2, O], U8, name="obs%d" % q)
+            nc.sync.dma_start(out=obs[q][:], in_=bytes_v[:, 2 * q:2 * q + 2, :])
 
         def load_b1():
-            nc.sync.dma_start(out=b1c[:], in_=b1.rearrange("(g p t) -> p g t", p=P, t=4))
+            nc.sync.dma_start(out=b1_cols[:], in_=b1.rearrange("(g p t) -> p g t", p=P, t=4))
 
         def load_b2():
-            nc.sync.dma_start(out=b2b[:], in_=b2.partition_broadcast(P))
+            nc.sync.dma_start(out=b2_rows[:], in_=b2.partition_broadcast(P))
 
         def load_eps():
             nc.sync.dma_start(out=eps_sb[:], in_=eps_v)
 
         def turn_scale():
-            tps["scale"] = psum.tile([P, 512], F32, name="tp")
-            nc.tensor.transpose(tps["scale"][:, :P], srow[:], ident[:])
+            banks["scale"] = psum.tile([P, P], F32, name="tp")
+            nc.tensor.transpose(banks["scale"][:], scale_rows[:], ident[:])
 
         def drain_scale():
-            nc.scalar.copy(out=scol[:], in_=tps["scale"][:, :SCALE_ROWS])
+            nc.scalar.copy(out=scale_cols[:], in_=banks["scale"][:, :SCALE_ROWS])
 
         def spread_scale(n):
-            tps["scale", n] = psum.tile([P, 4, P], F32, name="acc")
-            for c in range(4):
-                nc.tensor.transpose(tps["scale", n][:, c, :], scol[:, 4 * n + c:4 * n + c + 1].to_broadcast([P, P]), ident[:])
+            banks["scale", n] = psum.tile([P, 4, P], F32, name="acc")
+            for r in range(4):
+                column = scale_cols[:, 4 * n + r:4 * n + r + 1]
+                nc.tensor.transpose(banks["scale", n][:, r, :], column.to_broadcast([P, P]), ident[:])
 
         def drain_spread(n):
-            nc.scalar.copy(out=scale[:, 4 * SCALE_COLS * n:4 * SCALE_COLS * (n + 1)].rearrange("p (c k) -> p c k", c=4),
-                           in_=tps["scale", n][:, :, :SCALE_COLS])
+            out = scale[:, 4 * SCALE_COLS * n:4 * SCALE_COLS * (n + 1)].rearrange("p (r c) -> p r c", r=4)
+            nc.scalar.copy(out=out, in_=banks["scale", n][:, :, :SCALE_COLS])
 
-        def relus(b, half, t0):
-            relu(b, half, t0)
-            relu(b, half, t0 + 1)
+        def product(q, g):
+            k0 = max(KP * g, S + A)
+            c0, c1 = k0 - (S + A), KP * (g + 1) - (S + A)
+            for i in range(2):
+                nc.vector.tensor_tensor(out=row_tile(q, g)[:, i, k0 - KP * g:], in0=obs[q][:, i, c0:c1].bitcast(FP8),
+                                        in1=scale[:, c0:c1], op=ALU.mult)
 
-        def drain_x(b, n):
-            drain([(0, n), (1, n)] if b == 0 else [(b + 1, 2 * n), (b + 1, 2 * n + 1)])
+        def turn_tag(q, g):
+            return "acc" if (q, g // 2) == (3, 2) else "tp"
 
-        def quant_xn(b, n):
-            if b == 0:
-                quant_x(0, n, n + 1)
-            else:
-                quant_x(b, 2 * n, 2 * n + 2)
+        def turn(q, g):
+            banks[q, g] = psum.tile([P, 2, QT], F32, name=turn_tag(q, g))
+            for i in range(2):
+                words = rows[q, g][:, i, :].bitcast(F32)
+                for u in range(2):
+                    nc.tensor.transpose(banks[q, g][:, u, P * i:P * i + P], words[:, u::2], ident[:])
 
-        def weave_w1n(half, g):
-            weave_w1(half, g, True)
+        def bank_pair(n):
+            return [(0, n), (1, n)] if n < G1 else [(n // 3, 2 * (n % 3)), (n // 3, 2 * (n % 3) + 1)]
 
-        def weave_w1s(half, g):
-            weave_w1(half, g, False)
+        def pair_of(q, g):
+            return g if q < 2 else 3 * q + g // 2
 
-        w2_parts = [(g, c0) for g in range(G2) for c0 in (0, 512)]
+        def drain_x(n):
+            woven["x", n] = streamed("woven_s", [P, WOVEN], BF16)
+            for j, key in enumerate(bank_pair(n)):
+                out = woven["x", n][:].bitcast(F32)[:, KP * j:KP * j + KP].rearrange("p (r u) -> p r u", u=2)
+                nc.scalar.copy(out=out, in_=banks[key][:].rearrange("p u r -> p r u"))
 
-        def weave_w2n(n):
-            weave_w2(w2_parts[n][0], w2_parts[n][1], n in W2V)
+        def quant_x(n):
+            (q, g0), (q1, g1) = bank_pair(n)
+            grp = max(q1 - 1, 0)
+            nc.vector.quantize_mx(out=xc[grp][:, g0:g1 + 1, :].rearrange("p g n -> p (g n)").bitcast(FP8X4),
+                                  scales=xs[grp][:, g0:g1 + 1, :].rearrange("p g n -> p (g n)"), in_=woven["x", n][:])
 
-        def quant_w2n(n):
-            quant_w2(w2_parts[n][0], w2_parts[n][1])
+        def w1_shares(half, g):
+            cut = RUNS if (half, g) == (0, 0) else VECTOR_RUNS[half]
+            return {"vector": slice(0, cut), "scalar": slice(cut, RUNS)}
 
-        def weave_hn(b, half):
-            weave_h(b, half, (b, half) in HV)
+        def w1_weavers(half, g):
+            return [(weave_w1, half, g, e) for e, part in w1_shares(half, g).items() if part.stop > part.start]
 
-        def pair(b, half, t0):
-            hidden_pair(b, half, t0, "tp" if (b, half) == (1, 0) else "acc")
+        def weave_w1(half, g, engine):
+            if (half, g) not in woven:
+                woven[half, g] = streamed("woven_w", [P, WOVEN], BF16)
+            part = w1_shares(half, g)[engine]
+            copy[engine](out=woven[half, g][:].rearrange("p (s r e t) -> p r t e s", s=4, e=2, t=4)[:, part],
+                         in_=raw[half, g][:].rearrange("p t (r e s) -> p r t e s", e=2, s=4)[:, part])
 
-        block_of = [0, 0, 1, 2]
-        units = [G1, G1 // 2, G1 // 2]
+        def quant_w1(half, g):
+            cols = slice(KP * half, KP * half + KP)
+            nc.vector.quantize_mx(out=w1c[:, g, cols].bitcast(FP8X4), scales=w1s[:, g, cols], in_=woven[half, g][:])
 
-        def needs(step):
-            f, a = step[0], step[1:]
-            if f == turn_scale:
-                return [(load_scale,)]
-            if f == drain_scale:
-                return [(turn_scale,)]
-            if f == spread_scale:
-                return [(drain_scale,)]
-            if f == drain_spread:
-                return [(spread_scale, a[0])]
-            if f == product:
-                return [(load_obs, a[0])] + [(drain_spread, n) for n in range(a[1] - 1)]
-            if f == turn:
-                return [(load_state, a[0], a[1])] if a[1] < 2 else [(product, a[0], a[1])] + [(load_action, a[0])]
-            if f == drain_x:
-                return [(turn, 0, a[1]), (turn, 1, a[1])] if a[0] == 0 else [(turn, a[0] + 1, 2 * a[1]), (turn, a[0] + 1, 2 * a[1] + 1)]
-            if f == quant_xn:
-                return [(drain_x,) + a]
-            if f in (weave_w1n, weave_w1s):
-                return [(load_w1,) + a]
-            if f == quant_w1:
-                return [(weave_w1n,) + a] + ([(weave_w1s,) + a] if share(*a) < 64 else [])
-            if f == weave_w2n:
-                return [(load_w2, a[0] // 2)]
-            if f == quant_w2n:
-                return [(weave_w2n,) + a]
-            if f == hidden_pass:
-                return [(quant_w1, a[1], a[2]), (quant_xn, 0, a[2])] + ([(hidden_pass, 0, a[1], a[2] - 1)] if a[2] else [])
-            if f == pair:
-                return [(quant_w1, a[1], g) for g in range(G1)] + [(quant_xn, spans[a[0]][0], n) for n in range(3)]
-            if f == relus:
-                return [(load_b1,), (hidden_pass, 0, a[1], G1 - 1) if a[0] == 0 else (pair, a[0], a[1], a[2] if a[0] == 1 else 0)] + ([(relus, a[0], a[1], 0)] if a[2] else [])
-            if f == weave_hn:
-                return [(relus, a[0], a[1], 0), (relus, a[0], a[1], 2)]
-            if f == quant_h:
-                return [(weave_hn,) + a]
-            if f == heads:
-                return [(quant_h, span_of[a[0]], 0), (quant_h, span_of[a[0]], 1)] + [(quant_w2n, n) for n in range(4)]
-            if f == bias_wide:
-                return [(heads, a[0]), (load_b2,)]
-            if f in (bias_narrow, root, store_std):
-                return [(bias_wide,) + a]
-            if f == noise:
-                return [(root,) + a, (load_eps,)]
-            if f == shift:
-                return [(noise,) + a, (bias_narrow, a[0])]
-            if f == store_mean:
-                return [(bias_narrow,) + a]
-            if f == store_sample:
-                return [(shift,) + a]
-            return []
+        def weave(key, src, engine):
+            buf = streamed("woven_v" if engine == "vector" else "woven_s", [P, WOVEN], BF16)
+            woven[key] = buf[:, :4 * src.shape[2]]
+            copy[engine](out=woven[key].rearrange("p (r e t) -> p r t e", e=8, t=4),
+                         in_=src.rearrange("p t (r e) -> p r t e", e=8))
 
-        def takes(step):
-            f, a = step[0], step[1:]
-            woven = {True: "woven_v", False: "woven_s"}
-            if f == load_w1:
-                return [("wraw", 7, [(weave_w1n,) + a] + ([(weave_w1s,) + a] if share(*a) < 64 else []))]
-            if f == load_w2:
-                return [("wraw", 7, [(weave_w2n, 2 * a[0] + n)]) for n in range(2)]
-            if f in (load_state, product) and (a[0], a[1]) not in xr:
-                return [("xr%d" % a[1], 3, [(turn,) + a])]
-            if f == load_action and (a[0], 2) not in xr:
-                return [("xr2", 3, [(turn, a[0], 2)])]
-            if f == drain_x:
-                return [("woven_s", 3, [(quant_xn,) + a])]
-            if f in (weave_w1n, weave_w1s) and a not in wi:
-                return [("woven_w", 3, [(quant_w1,) + a])]
-            if f == weave_w2n:
-                return [(woven[a[0] in W2V], 2 if a[0] in W2V else 3, [(quant_w2n,) + a])]
-            if f == weave_hn:
-                return [(woven[a in HV], 2 if a in HV else 3, [(quant_h,) + a])]
-            if f == turn_scale:
-                return [("tp", 4, [(drain_scale,)])]
-            if f == spread_scale:
-                return [("acc", 4, [(drain_spread,) + a])]
-            if f == turn:
-                return [("tp", 4, [(drain_x, block_of[a[0]], a[1] if a[0] < 2 else a[1] // 2)])]
-            if f == hidden_pass and a[2] == 0:
-                return [("acc", 4, [(relus, 0, a[1], 2 * (t // 2))]) for t in range(4)]
-            if f == pair:
-                return [("tp" if a[:2] == (1, 0) else "acc", 4, [(relus, a[0], a[1], a[2] if a[0] == 1 else 2)])]
-            if f == relus and a[2] == 0:
-                return [("hp%d" % spans[a[0]][2], 2, [(weave_hn, a[0], a[1])])]
-            if f == heads:
-                return [("tp", 4, [(bias_wide, a[0])]), ("tp", 4, [(bias_narrow, a[0])])]
-            if f == bias_wide:
-                return [("res", 4, [(store_std,) + a, (store_mean,) + a, (store_sample,) + a])]
-            return []
+        def weave_w2(piece, engine):
+            weave(piece, raw[piece][:], engine)
+
+        def quant_w2(piece):
+            g, c0, n = piece
+            nc.vector.quantize_mx(out=w2c[:, g, c0:c0 + n].bitcast(FP8X4), scales=w2s[:, g, c0:c0 + n], in_=woven[piece])
+
+        def mm1(span, half, t, g):
+            grp, r0, n = span
+            cols = slice(KP * half + P * t, KP * half + P * t + P)
+            nc.tensor.matmul_mx(out=banks[span, half, t], lhsT=w1c[:, g, cols].bitcast(FP8X4), lhsT_scale=w1s[:, g, cols],
+                                rhs=xc[grp][:, g, r0:r0 + n].bitcast(FP8X4), rhs_scale=xs[grp][:, g, r0:r0 + n],
+                                start=(g == 0), stop=(g == G1 - 1))
+
+        def front_pass(half, g):
+            for t in range(4):
+                if g == 0:
+                    acc = psum.tile([P, KP], F32, name="acc")
+                    banks[FRONT, half, t] = acc[:]
+                mm1(FRONT, half, t, g)
+
+        def bank_tag(span, half):
+            return "tp" if (span, half) == (THIRD, 0) else "acc"
+
+        def bank_start(span, t):
+            return t - t % (KP // span[2])
+
+        def fill_bank(span, half, t0):
+            n = span[2]
+            acc = psum.tile([P, KP // n, n], F32, name=bank_tag(span, half))
+            for t in range(t0, t0 + KP // n):
+                banks[span, half, t] = acc[:, t - t0, :]
+                for g in range(G1):
+                    mm1(span, half, t, g)
+
+        def relu(span, half, t0):
+            n = span[2]
+            if t0 == 0:
+                hidden[span, half] = stream.tile([P, 4, n], BF16, name="hidden%d" % n, bufs=HIDDEN_DEPTH[n])
+            for t in (t0, t0 + 1):
+                nc.scalar.activation(hidden[span, half][:, t, :], banks[span, half, t], ACT.Relu,
+                                     bias=b1_cols[:, half, t:t + 1])
+
+        def weave_h(span, half, engine):
+            weave((span, half), hidden[span, half][:], engine)
+
+        def quant_h(span, half):
+            grp, r0, n = span
+            nc.vector.quantize_mx(out=hc[grp][:, half, r0:r0 + n].bitcast(FP8X4), scales=hs[grp][:, half, r0:r0 + n],
+                                  in_=woven[span, half])
+
+        def spans_of(n):
+            front, third = [(FRONT, 0), (FRONT, 1)], [(THIRD, 0), (THIRD, 1)]
+            return front if n < 4 else third if n < 6 else [(LAST, 0), ((LAST_A, LAST_B)[n - 6], 1)]
+
+        def heads(n):
+            grp = max(n // 2 - 1, 0)
+            r0 = P * (n - 2 * GROUPS[grp][0])
+            for c0, c1 in ((SPLIT, 2 * L), (0, SPLIT)):
+                banks["head", n, c0] = psum.tile([P, c1 - c0], F32, name="tp")
+                for g in range(G2):
+                    nc.tensor.matmul_mx(out=banks["head", n, c0][:], lhsT=hc[grp][:, g, r0:r0 + P].bitcast(FP8X4),
+                                        lhsT_scale=hs[grp][:, g, r0:r0 + P], rhs=w2c[:, g, c0:c1].bitcast(FP8X4),
+                                        rhs_scale=w2s[:, g, c0:c1], start=(g == 0), stop=(g == G2 - 1))
+
+        def bias_wide(n):
+            result[n] = streamed("res", [P, 2 * L], F32)
+            result[n, "sample"] = stream.tile([P, L], F32, name="sample", bufs=DEPTH["res"])
+            nc.vector.tensor_add(out=result[n][:, SPLIT:], in0=banks["head", n, SPLIT][:], in1=b2_rows[:, SPLIT:])
+
+        def bias_narrow(n):
+            nc.vector.tensor_add(out=result[n][:, :SPLIT], in0=banks["head", n, 0][:], in1=b2_rows[:, :SPLIT])
+
+        def root(n):
+            nc.scalar.activation(result[n, "sample"][:], result[n][:, L:], ACT.Sqrt)
+
+        def noise(n):
+            nc.vector.tensor_mul(out=result[n, "sample"][:], in0=result[n, "sample"][:], in1=eps_sb[:, n, :])
+
+        def shift(n):
+            nc.vector.tensor_add(out=result[n, "sample"][:], in0=result[n, "sample"][:], in1=result[n][:, :L])
+
+        def store_std(n):
+            nc.sync.dma_start(out=std_v[:, n, :], in_=result[n][:, L:])
+
+        def store_mean(n):
+            nc.sync.dma_start(out=mean_v[:, n, :], in_=result[n][:, :L])
+
+        def store_sample(n):
+            nc.sync.dma_start(out=sample_v[:, n, :], in_=result[n, "sample"][:])
 
         def rows_of(q):
             return [(load_obs, q), (load_state, q, 0), (load_state, q, 1), (load_action, q)]
 
-        def pair_of_turns(n):
-            return [(turn, 0, n), (turn, 1, n)] if n < G1 else [(turn, n // 3, 2 * (n % 3)), (turn, n // 3, 2 * (n % 3) + 1)]
+        def turns(n):
+            return [(turn, q, g) for q, g in bank_pair(n)]
 
-        def both_relus(b, half):
-            return [(relus, b, half, 0), (relus, b, half, 2)]
+        def relus(span, half):
+            return [(relu, span, half, 0), (relu, span, half, 2)]
 
-        small = [(2, 0), (2, 1), (3, 0), (3, 1)]
-
-        sync_q = [(load_scale,), (load_w1, 0, 0), (load_obs, 0), (load_state, 0, 0), (load_state, 1, 0), (load_w1, 0, 1),
-                  (load_obs, 1), (load_state, 0, 1), (load_state, 1, 1), (load_action, 0), (load_action, 1)]
-        sync_q += [(load_w1, 0, g) for g in range(2, G1)] + [(load_b1,)] + rows_of(2)
-        sync_q += [(load_w1, 1, g) for g in range(G1)] + rows_of(3)
-        sync_q += [(load_w2, 0), (load_w2, 1), (load_b2,), (load_eps,)]
+        sync_q = [(load_scale,), (load_w1, 0, 0), (load_obs, 0), (load_obs, 1), (load_w1, 0, 1)]
+        sync_q += [(load_state, q, g) for g in range(STATE_PASSES) for q in GROUPS[0]]
+        sync_q += [(load_action, q) for q in GROUPS[0]] + [(load_w1, 0, g) for g in range(2, G1)] + [(load_b1,)]
+        sync_q += rows_of(2) + [(load_w1, 1, g) for g in range(G1)] + rows_of(3)
+        sync_q += [(load_w2, piece) for piece in W2_PIECES] + [(load_b2,), (load_eps,)]
         for n in range(NT):
             sync_q += [(store_std, n), (store_mean, n)] + ([(store_sample, n - 1)] if n else [])
         sync_q += [(store_sample, NT - 1)]
 
-        tensor_q = [(turn_scale,)] + [(spread_scale, n) for n in range(4)]
+        tensor_q = [(turn_scale,)] + [(spread_scale, n) for n in range(SCALE_ROWS // 4)]
         for n in range(LEAD):
-            tensor_q += pair_of_turns(n)
+            tensor_q += turns(n)
         for g in range(G1):
-            tensor_q += [(hidden_pass, 0, 0, g)] + pair_of_turns(g + LEAD)
-        tensor_q += [(hidden_pass, 0, 1, 0), (pair, 1, 0, 0), (pair, 1, 0, 2)]
-        tensor_q += [(hidden_pass, 0, 1, g) for g in range(1, G1)]
-        tensor_q += pair_of_turns(9) + [(pair, 1, 1, 0)] + pair_of_turns(10) + [(pair, 1, 1, 2)] + pair_of_turns(11)
+            tensor_q += [(front_pass, 0, g)] + turns(g + LEAD)
+        tensor_q += [(front_pass, 1, 0), (fill_bank, THIRD, 0, 0), (fill_bank, THIRD, 0, 2)]
+        tensor_q += [(front_pass, 1, g) for g in range(1, G1)]
+        tensor_q += turns(9) + [(fill_bank, THIRD, 1, 0)] + turns(10) + turns(11) + [(fill_bank, THIRD, 1, 2)]
         tensor_q += [(heads, 0), (heads, 1)]
-        for n, (b, half) in enumerate(small):
-            tensor_q += [(heads, n + 2), (pair, b, half, 0)]
-        tensor_q += [(heads, 6), (heads, 7)]
+        for n, bank in enumerate(((LAST, 0, 0), (LAST, 0, 2), (LAST_A, 1, 0), (LAST_B, 1, 0))):
+            tensor_q += [(heads, n + 2), (fill_bank,) + bank]
+        tensor_q += [(heads, NT - 2), (heads, NT - 1)]
 
-        scalar_q = [(drain_scale,)] + [(drain_spread, n) for n in range(4)] + [(drain_x, 0, 0)]
+        scalar_q = [(drain_scale,)] + [(drain_spread, n) for n in range(SCALE_ROWS // 4)]
+        scalar_q += [(weave_w1, 0, 1, "scalar"), (drain_x, 0), (drain_x, 1)]
+        for g in range(2, G1):
+            scalar_q += [(weave_w1, 0, g, "scalar"), (drain_x, g)]
+        scalar_q += [(drain_x, 6), (weave_w1, 1, 0, "scalar"), (drain_x, 7)] + relus(FRONT, 0) + [(drain_x, 8)]
+        scalar_q += [(weave_w1, 1, g, "scalar") for g in range(1, G1)] + relus(THIRD, 0)
+        scalar_q += [(weave_w2, W2_PIECES[0], "scalar")] + relus(FRONT, 1) + [(weave_h, FRONT, 1, "scalar")]
+        scalar_q += [(drain_x, n) for n in (9, 10, 11)] + relus(THIRD, 1)
+        between_roots = [[(weave_h, THIRD, 0, "scalar")], [(weave_h, THIRD, 1, "scalar")], [(relu, LAST, 0, 0)],
+                         [(relu, LAST, 0, 2), (weave_h, LAST, 0, "scalar")],
+                         relus(LAST_A, 1) + [(weave_h, LAST_A, 1, "scalar")], relus(LAST_B, 1), [], []]
+        for n in range(NT):
+            scalar_q += [(root, n)] + between_roots[n]
+
+        products = [(product, q, g) for g in range(STATE_PASSES, G1) for q in GROUPS[0]]
+        products += [(product, q, g) for q in (2, 3) for g in range(STATE_PASSES, G1)]
+        vector_q = [(weave_w1, 0, 0, "vector"), products.pop(0), (quant_w1, 0, 0), products.pop(0), products.pop(0)]
+        vector_q += [(weave_w1, 0, 1, "vector"), products.pop(0), (quant_w1, 0, 1), (quant_x, 0), (quant_x, 1)]
+        for g in range(2, G1):
+            vector_q += [(weave_w1, 0, g, "vector"), products.pop(0), (quant_w1, 0, g)]
+            vector_q += ([products.pop(0)] if g + 2 < G1 else []) + [(quant_x, g)]
+        vector_q += [(weave_w1, 1, 0, "vector"), products.pop(0), (quant_w1, 1, 0), products.pop(0), (quant_x, 6)]
+        vector_q += [(weave_w1, 1, 1, "vector"), (quant_x, 7), (weave_w1, 1, 2, "vector"), (quant_x, 8)]
         for g in range(1, G1):
-            scalar_q += [(weave_w1s, 0, g), (drain_x, 0, g)]
-        scalar_q += [(drain_x, 1, 0), (weave_w1s, 1, 0), (drain_x, 1, 1)] + both_relus(0, 0) + [(drain_x, 1, 2)]
-        scalar_q += [(weave_w1s, 1, g) for g in range(1, G1)] + both_relus(1, 0) + [(weave_w2n, 0)]
-        scalar_q += both_relus(0, 1) + [(weave_hn, 0, 1)] + [(drain_x, 2, n) for n in range(3)] + both_relus(1, 1)
-        scalar_q += [(root, 0), (weave_hn, 1, 0), (root, 1), (weave_hn, 1, 1), (root, 2)]
-        for n, (b, half) in enumerate(small):
-            scalar_q += both_relus(b, half) + ([(weave_hn, b, half)] if (b, half) not in HV else []) + [(root, n + 3)]
-        scalar_q += [(root, 7)]
+            vector_q += [(quant_w1, 1, g), (weave_w1, 1, g + 2, "vector") if g + 2 < G1 else products.pop(0)]
+        vector_q += [(weave_h, FRONT, 0, "vector"), products.pop(0), (quant_h, FRONT, 0), products.pop(0)]
+        w2_order = [W2_PIECES[n] for n in (0, 2, 1, 3)]
+        for piece, following in zip(w2_order, w2_order[1:]):
+            vector_q += [(weave_w2, following, "vector"), (quant_w2, piece)]
+        vector_q += [(quant_w2, w2_order[-1]), (quant_h, FRONT, 1), (quant_x, 9), (quant_x, 10)]
+        after_tile = {0: [(quant_x, 11)], 2: [(quant_h, THIRD, 0), (quant_h, THIRD, 1)], 4: [(quant_h, LAST, 0)],
+                      5: [(quant_h, LAST_A, 1)]}
+        for n in range(NT - 2):
+            vector_q += [(bias_wide, n)] + ([(noise, n - 1)] if n else []) + [(bias_narrow, n)]
+            vector_q += ([(shift, n - 1)] if n else []) + after_tile.get(n, [])
+        vector_q += [(noise, 5), (weave_h, LAST_B, 1, "vector"), (shift, 5), (quant_h, LAST_B, 1)]
+        vector_q += [(bias_wide, 6), (bias_narrow, 6), (bias_wide, 7), (noise, 6), (bias_narrow, 7), (shift, 6)]
+        vector_q += [(noise, 7), (shift, 7)]
 
-        products = [(product, q, g) for g0 in (2, 4) for q, g in (((0, g0), (0, g0 + 1), (1, g0), (1, g0 + 1)) if g0 == 2 else ((0, 4), (1, 4), (0, 5), (1, 5)))]
-        products += [(product, q, g) for q in (2, 3) for g in range(2, G1)]
-        vector_q = []
-        for g in range(G1):
-            vector_q += [(weave_w1n, 0, g), products.pop(0), (quant_w1, 0, g)] + ([products.pop(0)] if g < 4 else []) + [(quant_xn, 0, g)]
-        vector_q += [(weave_w1n, 1, 0), products.pop(0), (quant_w1, 1, 0), products.pop(0), (quant_xn, 1, 0)]
-        vector_q += [(weave_w1n, 1, 1), (quant_xn, 1, 1), (weave_w1n, 1, 2), (quant_xn, 1, 2)]
-        for g in range(1, 4):
-            vector_q += [(quant_w1, 1, g), (weave_w1n, 1, g + 2)]
-        vector_q += [(quant_w1, 1, 4), products.pop(0), (quant_w1, 1, 5), products.pop(0)]
-        vector_q += [(weave_hn, 0, 0), products.pop(0), (quant_h, 0, 0), products.pop(0)]
-        for n, m in ((2, 0), (1, 2), (3, 1)):
-            vector_q += [(weave_w2n, n), (quant_w2n, m)]
-        vector_q += [(quant_w2n, 3), (quant_h, 0, 1), (quant_xn, 2, 0), (quant_xn, 2, 1)]
-        between = [[(quant_xn, 2, 2)], [(quant_h, 1, 0)], [(quant_h, 1, 1)], [(quant_h, 2, 0)], [(quant_h, 2, 1)], [(quant_h, 3, 0), (weave_hn, 3, 1)]]
-        for n in range(NT + 1):
-            vector_q += [(bias_wide, n)] if n < NT else []
-            vector_q += [(quant_h, 3, 1)] if n == 6 else []
-            vector_q += [(noise, n - 1)] if n else []
-            vector_q += [(bias_narrow, n)] if n < NT else []
-            vector_q += [(shift, n - 1)] if n else []
-            vector_q += between[n] if n < len(between) else []
-        done = set()
-        held = {}
+        weaver = {step[1:-1]: step for step in vector_q + scalar_q if step[0] in (weave_w2, weave_h)}
+
+        def needs(f, *a):
+            if f == product:
+                return [(load_obs, a[0])] + [(drain_spread, n) for n in range(a[1] - 1)]
+            if f == turn:
+                return [(load_state,) + a] if a[1] < STATE_PASSES else [(product,) + a, (load_action, a[0])]
+            if f == quant_w1:
+                return w1_weavers(*a)
+            if f == front_pass:
+                return [(quant_w1,) + a, (quant_x, a[1])]
+            if f == fill_bank:
+                quarter = GROUPS[a[0][0]][0]
+                return [(quant_w1, a[1], g) for g in range(G1)] + [(quant_x, pair_of(quarter, g)) for g in range(G1)]
+            if f == relu:
+                span, half, t0 = a
+                sums = (front_pass, half, G1 - 1) if span == FRONT else (fill_bank, span, half, bank_start(span, t0))
+                return [(load_b1,), sums]
+            if f == heads:
+                return [(quant_h,) + key for key in spans_of(a[0])] + [(quant_w2, piece) for piece in W2_PIECES]
+            simple = {turn_scale: [(load_scale,)], drain_scale: [(turn_scale,)], spread_scale: [(drain_scale,)],
+                      drain_spread: [(spread_scale,) + a], quant_x: [(drain_x,) + a],
+                      weave_w1: [(load_w1,) + a[:2]], weave_w2: [(load_w2,) + a[:1]],
+                      bias_wide: [(heads,) + a, (load_b2,)], bias_narrow: [(bias_wide,) + a], root: [(bias_wide,) + a],
+                      noise: [(root,) + a, (load_eps,)], shift: [(noise,) + a, (bias_narrow,) + a],
+                      store_std: [(bias_wide,) + a], store_mean: [(bias_narrow,) + a], store_sample: [(shift,) + a]}
+            if f in simple:
+                return simple[f]
+            if f == drain_x:
+                return turns(a[0])
+            if f == weave_h:
+                return relus(a[0], a[1])
+            if f in (quant_w2, quant_h):
+                return [weaver[a]]
+            return []
+
+        def takes(f, *a):
+            if f == load_w1:
+                return [("wraw", DEPTH["wraw"], w1_weavers(*a))]
+            if f == load_w2:
+                return [("wraw", DEPTH["wraw"], [weaver[a]])]
+            if f in (load_state, load_action, product):
+                key = a if f != load_action else (a[0], STATE_PASSES)
+                return [] if key in rows else [(("rows", key[1]), DEPTH["rows"], [(turn,) + key])]
+            if f == weave_w1:
+                return [] if a[:2] in woven else [("woven_w", DEPTH["woven_w"], [(quant_w1,) + a[:2]])]
+            if f in (weave_w2, weave_h):
+                tag = "woven_v" if a[-1] == "vector" else "woven_s"
+                return [(tag, DEPTH[tag], [(quant_w2 if f == weave_w2 else quant_h,) + a[:-1]])]
+            if f == drain_x:
+                return [("woven_s", DEPTH["woven_s"], [(quant_x,) + a])]
+            if f == turn_scale:
+                return [("tp", DEPTH["tp"], [(drain_scale,)])]
+            if f == spread_scale:
+                return [("acc", DEPTH["acc"], [(drain_spread,) + a])]
+            if f == turn:
+                return [(turn_tag(*a), DEPTH["tp"], [(drain_x, pair_of(*a))])]
+            if f == front_pass and a[1] == 0:
+                return [("acc", DEPTH["acc"], [(relu, FRONT, a[0], t - t % 2)]) for t in range(4)]
+            if f == fill_bank:
+                return [(bank_tag(a[0], a[1]), DEPTH["acc"], [(relu, a[0], a[1], a[2] + KP // a[0][2] - 2)])]
+            if f == relu and a[2] == 0:
+                return [(("hidden", a[0][2]), HIDDEN_DEPTH[a[0][2]], [weaver[a[:2]]])]
+            if f == heads:
+                return [("tp", DEPTH["tp"], [(bias_wide,) + a]), ("tp", DEPTH["tp"], [(bias_narrow,) + a])]
+            if f == bias_wide:
+                return [("res", DEPTH["res"], [(store_std,) + a, (store_mean,) + a, (store_sample,) + a])]
+            return []
+
+        nc.gpsimd.memset(scale_rows[:], 0.0)
+        make_identity(nc, ident[:])
+        nc.vector.memset(warm[:], 1.0)
+        nc.scalar.activation(warm[:], warm[:], ACT.Sqrt)
+
+        done, held = set(), {}
         queues = [sync_q, tensor_q, scalar_q, vector_q]
         while any(queues):
             moved = False
             for queue in queues:
-                if not queue or not all(n in done for n in needs(queue[0])):
+                if not queue or not all(other in done for other in needs(*queue[0])):
                     continue
-                slots = takes(queue[0])
-                count = {}
+                slots = takes(*queue[0])
+                taken = {tag: list(held.get(tag, [])) for tag, depth, readers in slots}
                 free = True
-                for tag, bufs, readers in slots:
-                    count[tag] = count.get(tag, 0) + 1
-                    n = len(held.get(tag, [])) + count[tag] - 1 - bufs
-                    free = free and (n < 0 or all(r in done for r in held[tag][n]))
-                if not free:
-                    continue
-                for tag, bufs, readers in slots:
-                    held.setdefault(tag, []).append(readers)
-                step = queue.pop(0)
-                step[0](*step[1:])
-                done.add(step)
-                moved = True
+                for tag, depth, readers in slots:
+                    previous = taken[tag][-depth] if len(taken[tag]) >= depth else []
+                    free = free and all(other in done for other in previous)
+                    taken[tag].append(readers)
+                if free:
+                    held.update(taken)
+                    step = queue.pop(0)
+                    step[0](*step[1:])
+                    done.add(step)
+                    moved = True
             assert moved

@@ -36,6 +36,7 @@ W2_PIECES = tuple((g, c0, min(KP, 2 * L - c0)) for g in range(G2) for c0 in (0, 
 RUNS = KP // 8
 VECTOR_RUNS = (18, 32)
 LEAD = 3
+VIA_TENSOR = ((1, 1),)
 DEPTH = {"wraw": 6, "woven_w": 3, "woven_v": 2, "woven_s": 4, "rows": 3, "res": 4, "acc": 4, "tp": 4}
 HIDDEN_DEPTH = {2 * QT: 2, QT: 3, P: 2}
 
@@ -76,6 +77,7 @@ def tile_rssm_pa_kernel(tc, prev_state, prev_action, obs_bytes, obs_scale, eps,
         b2_rows = keep.tile([P, 2 * L], BF16)
         eps_sb = keep.tile([P, NT, L], BF16)
         ident = keep.tile([P, P], F32)
+        ident_bf = keep.tile([P, P], BF16)
         warm = keep.tile([P, 1], F32)
 
         raw, woven, rows, obs, banks, hidden, result = {}, {}, {}, {}, {}, {}, {}
@@ -177,7 +179,9 @@ def tile_rssm_pa_kernel(tc, prev_state, prev_action, obs_bytes, obs_scale, eps,
             cut = RUNS if (half, g) == (0, 0) else VECTOR_RUNS[half]
             return {"vector": slice(0, cut), "scalar": slice(cut, RUNS)}
 
-        def w1_weavers(half, g):
+        def w1_weavers(half, g, by_tensor):
+            if (half, g) in VIA_TENSOR:
+                return [(by_tensor, half, g, k) for k in range(2)]
             return [(weave_w1, half, g, e) for e, part in w1_shares(half, g).items() if part.stop > part.start]
 
         def weave_w1(half, g, engine):
@@ -186,6 +190,20 @@ def tile_rssm_pa_kernel(tc, prev_state, prev_action, obs_bytes, obs_scale, eps,
             part = w1_shares(half, g)[engine]
             copy[engine](out=woven[half, g][:].rearrange("p (s r e t) -> p r t e s", s=4, e=2, t=4)[:, part],
                          in_=raw[half, g][:].rearrange("p t (r e s) -> p r t e s", e=2, s=4)[:, part])
+
+        def pass_w1(half, g, k):
+            banks["w", half, g, k] = psum.tile([P, 2, P, 4], BF16, name="tp")
+            for j in range(2):
+                c0 = 2 * P * k + P * j
+                nc.tensor.matmul(banks["w", half, g, k][:, j], ident_bf[:],
+                                 raw[half, g][:, :, c0:c0 + P].rearrange("p t c -> p c t"), start=True, stop=True)
+
+        def drain_w1(half, g, k):
+            if k == 0:
+                woven[half, g] = streamed("woven_s", [P, WOVEN], BF16)
+            out = woven[half, g][:].bitcast(F32).rearrange("p (s m w) -> p m s w", s=4, w=2)[:, 64 * k:64 * k + 64]
+            src = banks["w", half, g, k][:].rearrange("p j c t -> p (j c t)").bitcast(F32)
+            nc.scalar.copy(out=out, in_=src.rearrange("p (m s w) -> p m s w", s=4, w=2))
 
         def quant_w1(half, g):
             cols = slice(KP * half, KP * half + KP)
@@ -310,10 +328,10 @@ def tile_rssm_pa_kernel(tc, prev_state, prev_action, obs_bytes, obs_scale, eps,
         for n in range(LEAD):
             tensor_q += turns(n)
         for g in range(G1):
-            tensor_q += [(front_pass, 0, g)] + turns(g + LEAD)
+            tensor_q += [(front_pass, 0, g)] + ([(pass_w1, 1, 1, 0), (pass_w1, 1, 1, 1)] if g == G1 - 1 else []) + turns(g + LEAD)
         tensor_q += [(front_pass, 1, 0), (fill_bank, THIRD, 0, 0), (fill_bank, THIRD, 0, 2)]
         tensor_q += [(front_pass, 1, g) for g in range(1, G1)]
-        tensor_q += turns(9) + [(fill_bank, THIRD, 1, 0)] + turns(10) + turns(11) + [(fill_bank, THIRD, 1, 2)]
+        tensor_q += turns(9) + [(fill_bank, THIRD, 1, 0)] + turns(10) + [(fill_bank, THIRD, 1, 2)] + turns(11)
         tensor_q += [(heads, 0), (heads, 1)]
         for n, bank in enumerate(((LAST, 0, 0), (LAST, 0, 2), (LAST_A, 1, 0), (LAST_B, 1, 0))):
             tensor_q += [(heads, n + 2), (fill_bank,) + bank]
@@ -324,7 +342,8 @@ def tile_rssm_pa_kernel(tc, prev_state, prev_action, obs_bytes, obs_scale, eps,
         for g in range(2, G1):
             scalar_q += [(weave_w1, 0, g, "scalar"), (drain_x, g)]
         scalar_q += [(drain_x, 6), (weave_w1, 1, 0, "scalar"), (drain_x, 7)] + relus(FRONT, 0) + [(drain_x, 8)]
-        scalar_q += [(weave_w1, 1, g, "scalar") for g in range(1, G1)] + relus(THIRD, 0)
+        scalar_q += [(drain_w1, 1, 1, k) for k in range(2)]
+        scalar_q += [(weave_w1, 1, g, "scalar") for g in range(2, G1)] + relus(THIRD, 0)
         scalar_q += [(weave_w2, W2_PIECES[0], "scalar")] + relus(FRONT, 1) + [(weave_h, FRONT, 1, "scalar")]
         scalar_q += [(drain_x, n) for n in (9, 10, 11)] + relus(THIRD, 1)
         between_roots = [[(weave_h, THIRD, 0, "scalar")], [(weave_h, THIRD, 1, "scalar")], [(relu, LAST, 0, 0)],
@@ -341,10 +360,10 @@ def tile_rssm_pa_kernel(tc, prev_state, prev_action, obs_bytes, obs_scale, eps,
             vector_q += [(weave_w1, 0, g, "vector"), products.pop(0), (quant_w1, 0, g)]
             vector_q += ([products.pop(0)] if g + 2 < G1 else []) + [(quant_x, g)]
         vector_q += [(weave_w1, 1, 0, "vector"), products.pop(0), (quant_w1, 1, 0), products.pop(0), (quant_x, 6)]
-        vector_q += [(weave_w1, 1, 1, "vector"), (quant_x, 7), (weave_w1, 1, 2, "vector"), (quant_x, 8)]
+        vector_q += [(quant_x, 7), (weave_w1, 1, 2, "vector"), products.pop(0), (quant_x, 8)]
         for g in range(1, G1):
             vector_q += [(quant_w1, 1, g), (weave_w1, 1, g + 2, "vector") if g + 2 < G1 else products.pop(0)]
-        vector_q += [(weave_h, FRONT, 0, "vector"), products.pop(0), (quant_h, FRONT, 0), products.pop(0)]
+        vector_q += [(weave_h, FRONT, 0, "vector"), products.pop(0), (quant_h, FRONT, 0)]
         w2_order = [W2_PIECES[n] for n in (0, 2, 1, 3)]
         for piece, following in zip(w2_order, w2_order[1:]):
             vector_q += [(weave_w2, following, "vector"), (quant_w2, piece)]
@@ -366,7 +385,7 @@ def tile_rssm_pa_kernel(tc, prev_state, prev_action, obs_bytes, obs_scale, eps,
             if f == turn:
                 return [(load_state,) + a] if a[1] < STATE_PASSES else [(product,) + a, (load_action, a[0])]
             if f == quant_w1:
-                return w1_weavers(*a)
+                return w1_weavers(a[0], a[1], drain_w1)
             if f == front_pass:
                 return [(quant_w1,) + a, (quant_x, a[1])]
             if f == fill_bank:
@@ -380,7 +399,7 @@ def tile_rssm_pa_kernel(tc, prev_state, prev_action, obs_bytes, obs_scale, eps,
                 return [(quant_h,) + key for key in spans_of(a[0])] + [(quant_w2, piece) for piece in W2_PIECES]
             simple = {turn_scale: [(load_scale,)], drain_scale: [(turn_scale,)], spread_scale: [(drain_scale,)],
                       drain_spread: [(spread_scale,) + a], quant_x: [(drain_x,) + a],
-                      weave_w1: [(load_w1,) + a[:2]], weave_w2: [(load_w2,) + a[:1]],
+                      weave_w1: [(load_w1,) + a[:2]], pass_w1: [(load_w1,) + a[:2]], drain_w1: [(pass_w1,) + a], weave_w2: [(load_w2,) + a[:1]],
                       bias_wide: [(heads,) + a, (load_b2,)], bias_narrow: [(bias_wide,) + a], root: [(bias_wide,) + a],
                       noise: [(root,) + a, (load_eps,)], shift: [(noise,) + a, (bias_narrow,) + a],
                       store_std: [(bias_wide,) + a], store_mean: [(bias_narrow,) + a], store_sample: [(shift,) + a]}
@@ -396,7 +415,7 @@ def tile_rssm_pa_kernel(tc, prev_state, prev_action, obs_bytes, obs_scale, eps,
 
         def takes(f, *a):
             if f == load_w1:
-                return [("wraw", DEPTH["wraw"], w1_weavers(*a))]
+                return [("wraw", DEPTH["wraw"], w1_weavers(a[0], a[1], pass_w1))]
             if f == load_w2:
                 return [("wraw", DEPTH["wraw"], [weaver[a]])]
             if f in (load_state, load_action, product):
@@ -407,6 +426,10 @@ def tile_rssm_pa_kernel(tc, prev_state, prev_action, obs_bytes, obs_scale, eps,
             if f in (weave_w2, weave_h):
                 tag = "woven_v" if a[-1] == "vector" else "woven_s"
                 return [(tag, DEPTH[tag], [(quant_w2 if f == weave_w2 else quant_h,) + a[:-1]])]
+            if f == pass_w1:
+                return [("tp", DEPTH["tp"], [(drain_w1,) + a])]
+            if f == drain_w1 and a[2] == 0:
+                return [("woven_s", DEPTH["woven_s"], [(quant_w1,) + a[:2]])]
             if f == drain_x:
                 return [("woven_s", DEPTH["woven_s"], [(quant_x,) + a])]
             if f == turn_scale:
@@ -429,6 +452,7 @@ def tile_rssm_pa_kernel(tc, prev_state, prev_action, obs_bytes, obs_scale, eps,
 
         nc.gpsimd.memset(scale_rows[:], 0.0)
         make_identity(nc, ident[:])
+        make_identity(nc, ident_bf[:])
         nc.vector.memset(warm[:], 1.0)
         nc.scalar.activation(warm[:], warm[:], ACT.Sqrt)
 

@@ -34,7 +34,7 @@ SPLIT = 2 * L - KP
 W2_PIECES = tuple((g, c0, min(KP, 2 * L - c0)) for g in range(G2) for c0 in (0, KP))
 
 RUNS = KP // 8
-VECTOR_RUNS = (18, 32)
+VECTOR_RUNS = (14, 30)
 LEAD = 3
 VIA_TENSOR = ((1, 1),)
 DEPTH = {"wraw": 6, "woven_w": 3, "woven_v": 2, "woven_s": 4, "rows": 3, "res": 4, "acc": 4, "tp": 4}
@@ -101,11 +101,19 @@ def tile_rssm_pa_kernel(tc, prev_state, prev_action, obs_bytes, obs_scale, eps,
 
         def row_tile(q, g):
             if (q, g) not in rows:
-                rows[q, g] = stream.tile([P, 2, KP], BF16, name="rows%d" % g, bufs=DEPTH["rows"], align_bytes=64)
+                if q in GROUPS[0]:
+                    rows[q, g] = stream.tile([P, 2, KP], BF16, name="rows%d" % g, bufs=2, align_bytes=64)[:]
+                else:
+                    rows[q, g, "two"] = stream.tile([P, 2, 2 * KP], BF16, name="wide%d" % g, bufs=1, align_bytes=64)
+                    rows[q, g], rows[q, g + 1] = rows[q, g, "two"][:, :, :KP], rows[q, g, "two"][:, :, KP:]
             return rows[q, g]
 
         def load_state(q, g):
-            nc.sync.dma_start(out=row_tile(q, g)[:], in_=state_v[:, 2 * q:2 * q + 2, KP * g:KP * g + KP])
+            if q in GROUPS[0]:
+                nc.sync.dma_start(out=row_tile(q, g), in_=state_v[:, 2 * q:2 * q + 2, KP * g:KP * g + KP])
+            else:
+                row_tile(q, g)
+                nc.sync.dma_start(out=rows[q, g, "two"][:], in_=state_v[:, 2 * q:2 * q + 2, :])
 
         def load_action(q):
             nc.sync.dma_start(out=row_tile(q, STATE_PASSES)[:, :, :A], in_=action_v[:, 2 * q:2 * q + 2, :])
@@ -146,6 +154,13 @@ def tile_rssm_pa_kernel(tc, prev_state, prev_action, obs_bytes, obs_scale, eps,
             for i in range(2):
                 nc.vector.tensor_tensor(out=row_tile(q, g)[:, i, k0 - KP * g:], in0=obs[q][:, i, c0:c1].bitcast(FP8),
                                         in1=scale[:, c0:c1], op=ALU.mult)
+
+        def product_two(q, g, i):
+            k0 = max(KP * g, S + A)
+            c0, c1 = k0 - (S + A), KP * (g + 2) - (S + A)
+            row_tile(q, g)
+            nc.vector.tensor_tensor(out=rows[q, g, "two"][:, i, k0 - KP * g:], in0=obs[q][:, i, c0:c1].bitcast(FP8),
+                                    in1=scale[:, c0:c1], op=ALU.mult)
 
         def turn_tag(q, g):
             return "acc" if (q, g // 2) == (3, 2) else "tp"
@@ -270,12 +285,13 @@ def tile_rssm_pa_kernel(tc, prev_state, prev_action, obs_bytes, obs_scale, eps,
             front, third = [(FRONT, 0), (FRONT, 1)], [(THIRD, 0), (THIRD, 1)]
             return front if n < 4 else third if n < 6 else [(LAST, 0), ((LAST_A, LAST_B)[n - 6], 1)]
 
-        def heads(n):
+        def heads(n, passes=range(G2)):
             grp = max(n // 2 - 1, 0)
             r0 = P * (n - 2 * GROUPS[grp][0])
             for c0, c1 in ((SPLIT, 2 * L), (0, SPLIT)):
-                banks["head", n, c0] = psum.tile([P, c1 - c0], F32, name="tp")
-                for g in range(G2):
+                if 0 in passes:
+                    banks["head", n, c0] = psum.tile([P, c1 - c0], F32, name="tp")
+                for g in passes:
                     nc.tensor.matmul_mx(out=banks["head", n, c0][:], lhsT=hc[grp][:, g, r0:r0 + P].bitcast(FP8X4),
                                         lhsT_scale=hs[grp][:, g, r0:r0 + P], rhs=w2c[:, g, c0:c1].bitcast(FP8X4),
                                         rhs_scale=w2s[:, g, c0:c1], start=(g == 0), stop=(g == G2 - 1))
@@ -291,11 +307,13 @@ def tile_rssm_pa_kernel(tc, prev_state, prev_action, obs_bytes, obs_scale, eps,
         def root(n):
             nc.scalar.activation(result[n, "sample"][:], result[n][:, L:], ACT.Sqrt)
 
-        def noise(n):
-            nc.vector.tensor_mul(out=result[n, "sample"][:], in0=result[n, "sample"][:], in1=eps_sb[:, n, :])
+        def noise(n, c0=0, c1=L):
+            part = result[n, "sample"][:, c0:c1]
+            nc.vector.tensor_mul(out=part, in0=part, in1=eps_sb[:, n, c0:c1])
 
-        def shift(n):
-            nc.vector.tensor_add(out=result[n, "sample"][:], in0=result[n, "sample"][:], in1=result[n][:, :L])
+        def shift(n, c0=0, c1=L):
+            part = result[n, "sample"][:, c0:c1]
+            nc.vector.tensor_add(out=part, in0=part, in1=result[n][:, c0:c1])
 
         def store_std(n):
             nc.sync.dma_start(out=std_v[:, n, :], in_=result[n][:, L:])
@@ -303,11 +321,11 @@ def tile_rssm_pa_kernel(tc, prev_state, prev_action, obs_bytes, obs_scale, eps,
         def store_mean(n):
             nc.sync.dma_start(out=mean_v[:, n, :], in_=result[n][:, :L])
 
-        def store_sample(n):
-            nc.sync.dma_start(out=sample_v[:, n, :], in_=result[n, "sample"][:])
+        def store_sample(n, c0=0, c1=L):
+            nc.sync.dma_start(out=sample_v[:, n, c0:c1], in_=result[n, "sample"][:, c0:c1])
 
         def rows_of(q):
-            return [(load_obs, q), (load_state, q, 0), (load_state, q, 1), (load_action, q)]
+            return [(load_obs, q), (load_state, q, 0), (load_action, q)]
 
         def turns(n):
             return [(turn, q, g) for q, g in bank_pair(n)]
@@ -322,7 +340,8 @@ def tile_rssm_pa_kernel(tc, prev_state, prev_action, obs_bytes, obs_scale, eps,
         sync_q += [(load_w2, piece) for piece in W2_PIECES] + [(load_b2,), (load_eps,)]
         for n in range(NT):
             sync_q += [(store_std, n), (store_mean, n)] + ([(store_sample, n - 1)] if n else [])
-        sync_q += [(store_sample, NT - 1)]
+        halves = [(NT - 1, 0, L // 2), (NT - 1, L // 2, L)]
+        sync_q += [(store_sample,) + part for part in halves]
 
         tensor_q = [(turn_scale,)] + [(spread_scale, n) for n in range(SCALE_ROWS // 4)]
         for n in range(LEAD):
@@ -335,7 +354,7 @@ def tile_rssm_pa_kernel(tc, prev_state, prev_action, obs_bytes, obs_scale, eps,
         tensor_q += [(heads, 0), (heads, 1)]
         for n, bank in enumerate(((LAST, 0, 0), (LAST, 0, 2), (LAST_A, 1, 0), (LAST_B, 1, 0))):
             tensor_q += [(heads, n + 2), (fill_bank,) + bank]
-        tensor_q += [(heads, NT - 2), (heads, NT - 1)]
+        tensor_q += [(heads, NT - 2), (heads, NT - 1, (0,)), (heads, NT - 1, (1,))]
 
         scalar_q = [(drain_scale,)] + [(drain_spread, n) for n in range(SCALE_ROWS // 4)]
         scalar_q += [(weave_w1, 0, 1, "scalar"), (drain_x, 0), (drain_x, 1)]
@@ -353,14 +372,14 @@ def tile_rssm_pa_kernel(tc, prev_state, prev_action, obs_bytes, obs_scale, eps,
             scalar_q += [(root, n)] + between_roots[n]
 
         products = [(product, q, g) for g in range(STATE_PASSES, G1) for q in GROUPS[0]]
-        products += [(product, q, g) for q in (2, 3) for g in range(STATE_PASSES, G1)]
+        products += [(product_two, q, g, i) for q in (2, 3) for g in (2, 4) for i in range(2)]
         vector_q = [(weave_w1, 0, 0, "vector"), products.pop(0), (quant_w1, 0, 0), products.pop(0), products.pop(0)]
         vector_q += [(weave_w1, 0, 1, "vector"), products.pop(0), (quant_w1, 0, 1), (quant_x, 0), (quant_x, 1)]
         for g in range(2, G1):
             vector_q += [(weave_w1, 0, g, "vector"), products.pop(0), (quant_w1, 0, g)]
             vector_q += ([products.pop(0)] if g + 2 < G1 else []) + [(quant_x, g)]
         vector_q += [(weave_w1, 1, 0, "vector"), products.pop(0), (quant_w1, 1, 0), products.pop(0), (quant_x, 6)]
-        vector_q += [(quant_x, 7), (weave_w1, 1, 2, "vector"), products.pop(0), (quant_x, 8)]
+        vector_q += [(quant_x, 7), (weave_w1, 1, 2, "vector"), (quant_x, 8), products.pop(0)]
         for g in range(1, G1):
             vector_q += [(quant_w1, 1, g), (weave_w1, 1, g + 2, "vector") if g + 2 < G1 else products.pop(0)]
         vector_q += [(weave_h, FRONT, 0, "vector"), products.pop(0), (quant_h, FRONT, 0)]
@@ -375,13 +394,18 @@ def tile_rssm_pa_kernel(tc, prev_state, prev_action, obs_bytes, obs_scale, eps,
             vector_q += ([(shift, n - 1)] if n else []) + after_tile.get(n, [])
         vector_q += [(noise, 5), (weave_h, LAST_B, 1, "vector"), (shift, 5), (quant_h, LAST_B, 1)]
         vector_q += [(bias_wide, 6), (bias_narrow, 6), (bias_wide, 7), (noise, 6), (bias_narrow, 7), (shift, 6)]
-        vector_q += [(noise, 7), (shift, 7)]
+        vector_q += [(f,) + part for f in (noise, shift) for part in halves]
 
         weaver = {step[1:-1]: step for step in vector_q + scalar_q if step[0] in (weave_w2, weave_h)}
 
         def needs(f, *a):
             if f == product:
                 return [(load_obs, a[0])] + [(drain_spread, n) for n in range(a[1] - 1)]
+            if f == product_two:
+                return [(load_obs, a[0])]
+            if f == turn and a[0] not in GROUPS[0]:
+                g0 = a[1] - a[1] % 2
+                return [(load_state, a[0], 0)] if g0 == 0 else [(product_two, a[0], g0, i) for i in range(2)] + [(load_action, a[0])]
             if f == turn:
                 return [(load_state,) + a] if a[1] < STATE_PASSES else [(product,) + a, (load_action, a[0])]
             if f == quant_w1:
@@ -396,12 +420,12 @@ def tile_rssm_pa_kernel(tc, prev_state, prev_action, obs_bytes, obs_scale, eps,
                 sums = (front_pass, half, G1 - 1) if span == FRONT else (fill_bank, span, half, bank_start(span, t0))
                 return [(load_b1,), sums]
             if f == heads:
-                return [(quant_h,) + key for key in spans_of(a[0])] + [(quant_w2, piece) for piece in W2_PIECES]
+                return [(quant_h,) + key for key in spans_of(a[0]) if len(a) == 1 or key[1] in a[1]] + [(quant_w2, piece) for piece in W2_PIECES]
             simple = {turn_scale: [(load_scale,)], drain_scale: [(turn_scale,)], spread_scale: [(drain_scale,)],
                       drain_spread: [(spread_scale,) + a], quant_x: [(drain_x,) + a],
                       weave_w1: [(load_w1,) + a[:2]], pass_w1: [(load_w1,) + a[:2]], drain_w1: [(pass_w1,) + a], weave_w2: [(load_w2,) + a[:1]],
-                      bias_wide: [(heads,) + a, (load_b2,)], bias_narrow: [(bias_wide,) + a], root: [(bias_wide,) + a],
-                      noise: [(root,) + a, (load_eps,)], shift: [(noise,) + a, (bias_narrow,) + a],
+                      bias_wide: [(heads,) + a + ((1,),) * (a == (NT - 1,)), (load_b2,)], bias_narrow: [(bias_wide,) + a], root: [(bias_wide,) + a],
+                      noise: [(root,) + a[:1], (load_eps,)], shift: [(noise,) + a, (bias_narrow,) + a[:1]],
                       store_std: [(bias_wide,) + a], store_mean: [(bias_narrow,) + a], store_sample: [(shift,) + a]}
             if f in simple:
                 return simple[f]
@@ -418,9 +442,11 @@ def tile_rssm_pa_kernel(tc, prev_state, prev_action, obs_bytes, obs_scale, eps,
                 return [("wraw", DEPTH["wraw"], w1_weavers(a[0], a[1], pass_w1))]
             if f == load_w2:
                 return [("wraw", DEPTH["wraw"], [weaver[a]])]
-            if f in (load_state, load_action, product):
-                key = a if f != load_action else (a[0], STATE_PASSES)
-                return [] if key in rows else [(("rows", key[1]), DEPTH["rows"], [(turn,) + key])]
+            if f in (load_state, load_action, product, product_two):
+                key = a[:2] if f != load_action else (a[0], STATE_PASSES)
+                if a[0] not in GROUPS[0]:
+                    return [] if key in rows else [(("wide", key[1]), 1, [(turn,) + key, (turn, key[0], key[1] + 1)])]
+                return [] if key in rows else [(("rows", key[1]), 2, [(turn,) + key])]
             if f == weave_w1:
                 return [] if a[:2] in woven else [("woven_w", DEPTH["woven_w"], [(quant_w1,) + a[:2]])]
             if f in (weave_w2, weave_h):
@@ -444,8 +470,8 @@ def tile_rssm_pa_kernel(tc, prev_state, prev_action, obs_bytes, obs_scale, eps,
                 return [(bank_tag(a[0], a[1]), DEPTH["acc"], [(relu, a[0], a[1], a[2] + KP // a[0][2] - 2)])]
             if f == relu and a[2] == 0:
                 return [(("hidden", a[0][2]), HIDDEN_DEPTH[a[0][2]], [weaver[a[:2]]])]
-            if f == heads:
-                return [("tp", DEPTH["tp"], [(bias_wide,) + a]), ("tp", DEPTH["tp"], [(bias_narrow,) + a])]
+            if f == heads and a[1:] != ((1,),):
+                return [("tp", DEPTH["tp"], [(bias_wide, a[0])]), ("tp", DEPTH["tp"], [(bias_narrow, a[0])])]
             if f == bias_wide:
                 return [("res", DEPTH["res"], [(store_std,) + a, (store_mean,) + a, (store_sample,) + a])]
             return []

@@ -31,13 +31,15 @@ SCALE_COLS = O // SCALE_ROWS
 GROUPS = ((0, 1), (2,), (3,))
 FRONT, THIRD, LAST, LAST_A, LAST_B = (0, 0, 2 * QT), (1, 0, QT), (2, 0, QT), (2, 0, P), (2, P, P)
 SPLIT = 2 * L - KP
+ALL_PASSES, FIRST_PASS, SECOND_PASS = (0, 1), (0,), (1,)
 W2_PIECES = tuple((g, c0, min(KP, 2 * L - c0)) for g in range(G2) for c0 in (0, KP))
 
 RUNS = KP // 8
 VECTOR_RUNS = (14, 30)
 LEAD = 3
-VIA_TENSOR = ((1, 1),)
-DEPTH = {"wraw": 6, "woven_w": 3, "woven_v": 2, "woven_s": 4, "rows": 3, "res": 4, "acc": 4, "tp": 4}
+VIA_TENSOR = (1, 1)
+THIRD_X, LAST_X = (6, 7, 8), (9, 10, 11)
+DEPTH = {"wraw": 6, "woven_w": 3, "woven_v": 2, "woven_s": 4, "res": 4, "acc": 4, "tp": 4}
 HIDDEN_DEPTH = {2 * QT: 2, QT: 3, P: 2}
 
 
@@ -78,7 +80,6 @@ def tile_rssm_pa_kernel(tc, prev_state, prev_action, obs_bytes, obs_scale, eps,
         eps_sb = keep.tile([P, NT, L], BF16)
         ident = keep.tile([P, P], F32)
         ident_bf = keep.tile([P, P], BF16)
-        warm = keep.tile([P, 1], F32)
 
         raw, woven, rows, obs, banks, hidden, result = {}, {}, {}, {}, {}, {}, {}
         copy = {"vector": nc.vector.tensor_copy, "scalar": nc.scalar.copy}
@@ -99,21 +100,24 @@ def tile_rssm_pa_kernel(tc, prev_state, prev_action, obs_bytes, obs_scale, eps,
             raw[piece] = streamed("wraw", [P, 4, n], BF16)
             nc.sync.dma_start(out=raw[piece][:], in_=w2_v[g][:, :, c0:c0 + n])
 
+        def passes_in_tile(q):
+            return 1 if q in GROUPS[0] else 2
+
+        def rows_depth(q):
+            return 2 if q in GROUPS[0] else 1
+
         def row_tile(q, g):
             if (q, g) not in rows:
-                if q in GROUPS[0]:
-                    rows[q, g] = stream.tile([P, 2, KP], BF16, name="rows%d" % g, bufs=2, align_bytes=64)[:]
-                else:
-                    rows[q, g, "two"] = stream.tile([P, 2, 2 * KP], BF16, name="wide%d" % g, bufs=1, align_bytes=64)
-                    rows[q, g], rows[q, g + 1] = rows[q, g, "two"][:, :, :KP], rows[q, g, "two"][:, :, KP:]
-            return rows[q, g]
+                n = passes_in_tile(q)
+                buf = stream.tile([P, 2, n * KP], BF16, name=("rows%d" if n == 1 else "wide%d") % g, bufs=rows_depth(q), align_bytes=64)
+                rows[q, g, "tile"] = buf
+                for j in range(n):
+                    rows[q, g + j] = buf[:, :, KP * j:KP * j + KP]
+            return rows[q, g, "tile"]
 
         def load_state(q, g):
-            if q in GROUPS[0]:
-                nc.sync.dma_start(out=row_tile(q, g), in_=state_v[:, 2 * q:2 * q + 2, KP * g:KP * g + KP])
-            else:
-                row_tile(q, g)
-                nc.sync.dma_start(out=rows[q, g, "two"][:], in_=state_v[:, 2 * q:2 * q + 2, :])
+            k1 = KP * (g + passes_in_tile(q))
+            nc.sync.dma_start(out=row_tile(q, g)[:], in_=state_v[:, 2 * q:2 * q + 2, KP * g:k1])
 
         def load_action(q):
             nc.sync.dma_start(out=row_tile(q, STATE_PASSES)[:, :, :A], in_=action_v[:, 2 * q:2 * q + 2, :])
@@ -148,22 +152,18 @@ def tile_rssm_pa_kernel(tc, prev_state, prev_action, obs_bytes, obs_scale, eps,
             out = scale[:, 4 * SCALE_COLS * n:4 * SCALE_COLS * (n + 1)].rearrange("p (r c) -> p r c", r=4)
             nc.scalar.copy(out=out, in_=banks["scale", n][:, :, :SCALE_COLS])
 
-        def product(q, g):
+        def product(q, g, tiles):
             k0 = max(KP * g, S + A)
-            c0, c1 = k0 - (S + A), KP * (g + 1) - (S + A)
-            for i in range(2):
+            c0, c1 = k0 - (S + A), KP * (g + passes_in_tile(q)) - (S + A)
+            for i in tiles:
                 nc.vector.tensor_tensor(out=row_tile(q, g)[:, i, k0 - KP * g:], in0=obs[q][:, i, c0:c1].bitcast(FP8),
                                         in1=scale[:, c0:c1], op=ALU.mult)
 
-        def product_two(q, g, i):
-            k0 = max(KP * g, S + A)
-            c0, c1 = k0 - (S + A), KP * (g + 2) - (S + A)
-            row_tile(q, g)
-            nc.vector.tensor_tensor(out=rows[q, g, "two"][:, i, k0 - KP * g:], in0=obs[q][:, i, c0:c1].bitcast(FP8),
-                                    in1=scale[:, c0:c1], op=ALU.mult)
+        def product_steps(q, g):
+            return [(product, q, g, (0, 1))] if q in GROUPS[0] else [(product, q, g, (i,)) for i in range(2)]
 
         def turn_tag(q, g):
-            return "acc" if (q, g // 2) == (3, 2) else "tp"
+            return "acc" if pair_of(q, g) == LAST_X[2] else "tp"
 
         def turn(q, g):
             banks[q, g] = psum.tile([P, 2, QT], F32, name=turn_tag(q, g))
@@ -176,7 +176,7 @@ def tile_rssm_pa_kernel(tc, prev_state, prev_action, obs_bytes, obs_scale, eps,
             return [(0, n), (1, n)] if n < G1 else [(n // 3, 2 * (n % 3)), (n // 3, 2 * (n % 3) + 1)]
 
         def pair_of(q, g):
-            return g if q < 2 else 3 * q + g // 2
+            return g if q in GROUPS[0] else 3 * q + g // 2
 
         def drain_x(n):
             woven["x", n] = streamed("woven_s", [P, WOVEN], BF16)
@@ -185,8 +185,8 @@ def tile_rssm_pa_kernel(tc, prev_state, prev_action, obs_bytes, obs_scale, eps,
                 nc.scalar.copy(out=out, in_=banks[key][:].rearrange("p u r -> p r u"))
 
         def quant_x(n):
-            (q, g0), (q1, g1) = bank_pair(n)
-            grp = max(q1 - 1, 0)
+            g0, (q, g1) = bank_pair(n)[0][1], bank_pair(n)[1]
+            grp = max(q - 1, 0)
             nc.vector.quantize_mx(out=xc[grp][:, g0:g1 + 1, :].rearrange("p g n -> p (g n)").bitcast(FP8X4),
                                   scales=xs[grp][:, g0:g1 + 1, :].rearrange("p g n -> p (g n)"), in_=woven["x", n][:])
 
@@ -195,7 +195,7 @@ def tile_rssm_pa_kernel(tc, prev_state, prev_action, obs_bytes, obs_scale, eps,
             return {"vector": slice(0, cut), "scalar": slice(cut, RUNS)}
 
         def w1_weavers(half, g, by_tensor):
-            if (half, g) in VIA_TENSOR:
+            if (half, g) == VIA_TENSOR:
                 return [(by_tensor, half, g, k) for k in range(2)]
             return [(weave_w1, half, g, e) for e, part in w1_shares(half, g).items() if part.stop > part.start]
 
@@ -216,7 +216,8 @@ def tile_rssm_pa_kernel(tc, prev_state, prev_action, obs_bytes, obs_scale, eps,
         def drain_w1(half, g, k):
             if k == 0:
                 woven[half, g] = streamed("woven_s", [P, WOVEN], BF16)
-            out = woven[half, g][:].bitcast(F32).rearrange("p (s m w) -> p m s w", s=4, w=2)[:, 64 * k:64 * k + 64]
+            m0 = 2 * P * k // 4
+            out = woven[half, g][:].bitcast(F32).rearrange("p (s m w) -> p m s w", s=4, w=2)[:, m0:m0 + 2 * P // 4]
             src = banks["w", half, g, k][:].rearrange("p j c t -> p (j c t)").bitcast(F32)
             nc.scalar.copy(out=out, in_=src.rearrange("p (m s w) -> p m s w", s=4, w=2))
 
@@ -285,7 +286,7 @@ def tile_rssm_pa_kernel(tc, prev_state, prev_action, obs_bytes, obs_scale, eps,
             front, third = [(FRONT, 0), (FRONT, 1)], [(THIRD, 0), (THIRD, 1)]
             return front if n < 4 else third if n < 6 else [(LAST, 0), ((LAST_A, LAST_B)[n - 6], 1)]
 
-        def heads(n, passes=range(G2)):
+        def heads(n, passes=ALL_PASSES):
             grp = max(n // 2 - 1, 0)
             r0 = P * (n - 2 * GROUPS[grp][0])
             for c0, c1 in ((SPLIT, 2 * L), (0, SPLIT)):
@@ -347,51 +348,54 @@ def tile_rssm_pa_kernel(tc, prev_state, prev_action, obs_bytes, obs_scale, eps,
         for n in range(LEAD):
             tensor_q += turns(n)
         for g in range(G1):
-            tensor_q += [(front_pass, 0, g)] + ([(pass_w1, 1, 1, 0), (pass_w1, 1, 1, 1)] if g == G1 - 1 else []) + turns(g + LEAD)
+            tensor_q += [(front_pass, 0, g)] + (w1_weavers(*VIA_TENSOR, pass_w1) if g == G1 - 1 else [])
+            tensor_q += turns(g + LEAD)
         tensor_q += [(front_pass, 1, 0), (fill_bank, THIRD, 0, 0), (fill_bank, THIRD, 0, 2)]
         tensor_q += [(front_pass, 1, g) for g in range(1, G1)]
-        tensor_q += turns(9) + [(fill_bank, THIRD, 1, 0)] + turns(10) + [(fill_bank, THIRD, 1, 2)] + turns(11)
-        tensor_q += [(heads, 0), (heads, 1)]
+        tensor_q += turns(LAST_X[0]) + [(fill_bank, THIRD, 1, 0)] + turns(LAST_X[1])
+        tensor_q += [(fill_bank, THIRD, 1, 2)] + turns(LAST_X[2]) + [(heads, 0), (heads, 1)]
         for n, bank in enumerate(((LAST, 0, 0), (LAST, 0, 2), (LAST_A, 1, 0), (LAST_B, 1, 0))):
             tensor_q += [(heads, n + 2), (fill_bank,) + bank]
-        tensor_q += [(heads, NT - 2), (heads, NT - 1, (0,)), (heads, NT - 1, (1,))]
+        tensor_q += [(heads, NT - 2), (heads, NT - 1, FIRST_PASS), (heads, NT - 1, SECOND_PASS)]
 
         scalar_q = [(drain_scale,)] + [(drain_spread, n) for n in range(SCALE_ROWS // 4)]
         scalar_q += [(weave_w1, 0, 1, "scalar"), (drain_x, 0), (drain_x, 1)]
         for g in range(2, G1):
             scalar_q += [(weave_w1, 0, g, "scalar"), (drain_x, g)]
-        scalar_q += [(drain_x, 6), (weave_w1, 1, 0, "scalar"), (drain_x, 7)] + relus(FRONT, 0) + [(drain_x, 8)]
-        scalar_q += [(drain_w1, 1, 1, k) for k in range(2)]
-        scalar_q += [(weave_w1, 1, g, "scalar") for g in range(2, G1)] + relus(THIRD, 0)
+        scalar_q += [(drain_x, THIRD_X[0]), (weave_w1, 1, 0, "scalar"), (drain_x, THIRD_X[1])]
+        scalar_q += relus(FRONT, 0) + [(drain_x, THIRD_X[2])]
+        scalar_q += w1_weavers(*VIA_TENSOR, drain_w1) + [(weave_w1, 1, g, "scalar") for g in range(2, G1)]
+        scalar_q += relus(THIRD, 0)
         scalar_q += [(weave_w2, W2_PIECES[0], "scalar")] + relus(FRONT, 1) + [(weave_h, FRONT, 1, "scalar")]
-        scalar_q += [(drain_x, n) for n in (9, 10, 11)] + relus(THIRD, 1)
-        between_roots = [[(weave_h, THIRD, 0, "scalar")], [(weave_h, THIRD, 1, "scalar")], [(relu, LAST, 0, 0)],
-                         [(relu, LAST, 0, 2), (weave_h, LAST, 0, "scalar")],
-                         relus(LAST_A, 1) + [(weave_h, LAST_A, 1, "scalar")], relus(LAST_B, 1), [], []]
+        scalar_q += [(drain_x, n) for n in LAST_X] + relus(THIRD, 1)
+        after_root = [[(weave_h, THIRD, 0, "scalar")], [(weave_h, THIRD, 1, "scalar")], [(relu, LAST, 0, 0)],
+                      [(relu, LAST, 0, 2), (weave_h, LAST, 0, "scalar")],
+                      relus(LAST_A, 1) + [(weave_h, LAST_A, 1, "scalar")], relus(LAST_B, 1), [], []]
         for n in range(NT):
-            scalar_q += [(root, n)] + between_roots[n]
+            scalar_q += [(root, n)] + after_root[n]
 
-        products = [(product, q, g) for g in range(STATE_PASSES, G1) for q in GROUPS[0]]
-        products += [(product_two, q, g, i) for q in (2, 3) for g in (2, 4) for i in range(2)]
+        products = [step for g in range(STATE_PASSES, G1) for q in GROUPS[0] for step in product_steps(q, g)]
+        products += [step for q in (2, 3) for g in range(STATE_PASSES, G1, 2) for step in product_steps(q, g)]
         vector_q = [(weave_w1, 0, 0, "vector"), products.pop(0), (quant_w1, 0, 0), products.pop(0), products.pop(0)]
         vector_q += [(weave_w1, 0, 1, "vector"), products.pop(0), (quant_w1, 0, 1), (quant_x, 0), (quant_x, 1)]
         for g in range(2, G1):
             vector_q += [(weave_w1, 0, g, "vector"), products.pop(0), (quant_w1, 0, g)]
-            vector_q += ([products.pop(0)] if g + 2 < G1 else []) + [(quant_x, g)]
-        vector_q += [(weave_w1, 1, 0, "vector"), products.pop(0), (quant_w1, 1, 0), products.pop(0), (quant_x, 6)]
-        vector_q += [(quant_x, 7), (weave_w1, 1, 2, "vector"), (quant_x, 8), products.pop(0)]
+            vector_q += ([products.pop(0)] if g + STATE_PASSES < G1 else []) + [(quant_x, g)]
+        vector_q += [(weave_w1, 1, 0, "vector"), products.pop(0), (quant_w1, 1, 0), products.pop(0)]
+        vector_q += [(quant_x, THIRD_X[0]), (quant_x, THIRD_X[1]), (weave_w1, 1, 2, "vector")]
+        vector_q += [(quant_x, THIRD_X[2]), products.pop(0)]
         for g in range(1, G1):
             vector_q += [(quant_w1, 1, g), (weave_w1, 1, g + 2, "vector") if g + 2 < G1 else products.pop(0)]
         vector_q += [(weave_h, FRONT, 0, "vector"), products.pop(0), (quant_h, FRONT, 0)]
-        w2_order = [W2_PIECES[n] for n in (0, 2, 1, 3)]
+        w2_order = W2_PIECES[0::2] + W2_PIECES[1::2]
         for piece, following in zip(w2_order, w2_order[1:]):
             vector_q += [(weave_w2, following, "vector"), (quant_w2, piece)]
-        vector_q += [(quant_w2, w2_order[-1]), (quant_h, FRONT, 1), (quant_x, 9), (quant_x, 10)]
-        after_tile = {0: [(quant_x, 11)], 2: [(quant_h, THIRD, 0), (quant_h, THIRD, 1)], 4: [(quant_h, LAST, 0)],
-                      5: [(quant_h, LAST_A, 1)]}
+        vector_q += [(quant_w2, w2_order[-1]), (quant_h, FRONT, 1), (quant_x, LAST_X[0]), (quant_x, LAST_X[1])]
+        after_tile = [[(quant_x, LAST_X[2])], [], [(quant_h, THIRD, 0), (quant_h, THIRD, 1)], [],
+                      [(quant_h, LAST, 0)], [(quant_h, LAST_A, 1)]]
         for n in range(NT - 2):
             vector_q += [(bias_wide, n)] + ([(noise, n - 1)] if n else []) + [(bias_narrow, n)]
-            vector_q += ([(shift, n - 1)] if n else []) + after_tile.get(n, [])
+            vector_q += ([(shift, n - 1)] if n else []) + after_tile[n]
         vector_q += [(noise, 5), (weave_h, LAST_B, 1, "vector"), (shift, 5), (quant_h, LAST_B, 1)]
         vector_q += [(bias_wide, 6), (bias_narrow, 6), (bias_wide, 7), (noise, 6), (bias_narrow, 7), (shift, 6)]
         vector_q += [(f,) + part for f in (noise, shift) for part in halves]
@@ -401,13 +405,9 @@ def tile_rssm_pa_kernel(tc, prev_state, prev_action, obs_bytes, obs_scale, eps,
         def needs(f, *a):
             if f == product:
                 return [(load_obs, a[0])] + [(drain_spread, n) for n in range(a[1] - 1)]
-            if f == product_two:
-                return [(load_obs, a[0])]
-            if f == turn and a[0] not in GROUPS[0]:
-                g0 = a[1] - a[1] % 2
-                return [(load_state, a[0], 0)] if g0 == 0 else [(product_two, a[0], g0, i) for i in range(2)] + [(load_action, a[0])]
             if f == turn:
-                return [(load_state,) + a] if a[1] < STATE_PASSES else [(product,) + a, (load_action, a[0])]
+                q, g = a[0], a[1] - a[1] % passes_in_tile(a[0])
+                return [(load_state, q, g)] if g < STATE_PASSES else product_steps(q, g) + [(load_action, q)]
             if f == quant_w1:
                 return w1_weavers(a[0], a[1], drain_w1)
             if f == front_pass:
@@ -420,33 +420,34 @@ def tile_rssm_pa_kernel(tc, prev_state, prev_action, obs_bytes, obs_scale, eps,
                 sums = (front_pass, half, G1 - 1) if span == FRONT else (fill_bank, span, half, bank_start(span, t0))
                 return [(load_b1,), sums]
             if f == heads:
-                return [(quant_h,) + key for key in spans_of(a[0]) if len(a) == 1 or key[1] in a[1]] + [(quant_w2, piece) for piece in W2_PIECES]
-            simple = {turn_scale: [(load_scale,)], drain_scale: [(turn_scale,)], spread_scale: [(drain_scale,)],
-                      drain_spread: [(spread_scale,) + a], quant_x: [(drain_x,) + a],
-                      weave_w1: [(load_w1,) + a[:2]], pass_w1: [(load_w1,) + a[:2]], drain_w1: [(pass_w1,) + a], weave_w2: [(load_w2,) + a[:1]],
-                      bias_wide: [(heads,) + a + ((1,),) * (a == (NT - 1,)), (load_b2,)], bias_narrow: [(bias_wide,) + a], root: [(bias_wide,) + a],
-                      noise: [(root,) + a[:1], (load_eps,)], shift: [(noise,) + a, (bias_narrow,) + a[:1]],
-                      store_std: [(bias_wide,) + a], store_mean: [(bias_narrow,) + a], store_sample: [(shift,) + a]}
-            if f in simple:
-                return simple[f]
+                passes = a[1] if len(a) > 1 else ALL_PASSES
+                pieces = [(quant_h, span, half) for span, half in spans_of(a[0]) if half in passes]
+                return pieces + [(quant_w2, piece) for piece in W2_PIECES]
+            if f == bias_wide:
+                return [(heads, a[0], SECOND_PASS) if a[0] == NT - 1 else (heads, a[0]), (load_b2,)]
             if f == drain_x:
                 return turns(a[0])
             if f == weave_h:
                 return relus(a[0], a[1])
             if f in (quant_w2, quant_h):
                 return [weaver[a]]
-            return []
+            simple = {turn_scale: [(load_scale,)], drain_scale: [(turn_scale,)], spread_scale: [(drain_scale,)],
+                      drain_spread: [(spread_scale,) + a], quant_x: [(drain_x,) + a],
+                      weave_w1: [(load_w1,) + a[:2]], pass_w1: [(load_w1,) + a[:2]], drain_w1: [(pass_w1,) + a],
+                      weave_w2: [(load_w2,) + a[:1]], bias_narrow: [(bias_wide,) + a], root: [(bias_wide,) + a],
+                      noise: [(root,) + a[:1], (load_eps,)], shift: [(noise,) + a, (bias_narrow,) + a[:1]],
+                      store_std: [(bias_wide,) + a], store_mean: [(bias_narrow,) + a], store_sample: [(shift,) + a]}
+            return simple.get(f, [])
 
         def takes(f, *a):
             if f == load_w1:
                 return [("wraw", DEPTH["wraw"], w1_weavers(a[0], a[1], pass_w1))]
             if f == load_w2:
                 return [("wraw", DEPTH["wraw"], [weaver[a]])]
-            if f in (load_state, load_action, product, product_two):
-                key = a[:2] if f != load_action else (a[0], STATE_PASSES)
-                if a[0] not in GROUPS[0]:
-                    return [] if key in rows else [(("wide", key[1]), 1, [(turn,) + key, (turn, key[0], key[1] + 1)])]
-                return [] if key in rows else [(("rows", key[1]), 2, [(turn,) + key])]
+            if f in (load_state, load_action, product):
+                q, g = a[:2] if f != load_action else (a[0], STATE_PASSES)
+                n = passes_in_tile(q)
+                return [] if (q, g) in rows else [(("rows", n, g), rows_depth(q), [(turn, q, g + j) for j in range(n)])]
             if f == weave_w1:
                 return [] if a[:2] in woven else [("woven_w", DEPTH["woven_w"], [(quant_w1,) + a[:2]])]
             if f in (weave_w2, weave_h):
@@ -470,7 +471,7 @@ def tile_rssm_pa_kernel(tc, prev_state, prev_action, obs_bytes, obs_scale, eps,
                 return [(bank_tag(a[0], a[1]), DEPTH["acc"], [(relu, a[0], a[1], a[2] + KP // a[0][2] - 2)])]
             if f == relu and a[2] == 0:
                 return [(("hidden", a[0][2]), HIDDEN_DEPTH[a[0][2]], [weaver[a[:2]]])]
-            if f == heads and a[1:] != ((1,),):
+            if f == heads and a[1:] != (SECOND_PASS,):
                 return [("tp", DEPTH["tp"], [(bias_wide, a[0])]), ("tp", DEPTH["tp"], [(bias_narrow, a[0])])]
             if f == bias_wide:
                 return [("res", DEPTH["res"], [(store_std,) + a, (store_mean,) + a, (store_sample,) + a])]
@@ -478,9 +479,7 @@ def tile_rssm_pa_kernel(tc, prev_state, prev_action, obs_bytes, obs_scale, eps,
 
         nc.gpsimd.memset(scale_rows[:], 0.0)
         make_identity(nc, ident[:])
-        make_identity(nc, ident_bf[:])
-        nc.vector.memset(warm[:], 1.0)
-        nc.scalar.activation(warm[:], warm[:], ACT.Sqrt)
+        nc.scalar.activation(ident_bf[:], ident[:], ACT.Sqrt)
 
         done, held = set(), {}
         queues = [sync_q, tensor_q, scalar_q, vector_q]

@@ -24,22 +24,17 @@ NT = B // P
 QT = 2 * P
 STATE_PASSES = S // KP
 WOVEN = 4 * KP
-
-SCALE_ROWS = 16
-SCALE_COLS = O // SCALE_ROWS
+ACTION_ROWS = A // 4
 
 GROUPS = ((0, 1), (2,), (3,))
 FRONT, THIRD, LAST, LAST_A, LAST_B = (0, 0, 2 * QT), (1, 0, QT), (2, 0, QT), (2, 0, P), (2, P, P)
 SPLIT = 2 * L - KP
 ALL_PASSES, FIRST_PASS, SECOND_PASS = (0, 1), (0,), (1,)
 W2_PIECES = tuple((g, c0, min(KP, 2 * L - c0)) for g in range(G2) for c0 in (0, KP))
-
 RUNS = KP // 8
-VECTOR_RUNS = (14, 30)
-LEAD = 3
-VIA_TENSOR = (1, 1)
-THIRD_X, LAST_X = (6, 7, 8), (9, 10, 11)
-DEPTH = {"wraw": 6, "woven_w": 3, "woven_v": 2, "woven_s": 4, "res": 4, "acc": 4, "tp": 4}
+ORDER = (4, 5, 0, 2, 1, 3)
+DEPTH = {"wraw": 7, "woven_w": 3, "woven_g": 1, "woven_v": 1, "woven_s": 2, "woven_x": 3, "res": 4,
+         "state1": 4, "state2": 1, "wide2": 8, "wide4": 4, "obs2": 2, "obs4": 2}
 HIDDEN_DEPTH = {2 * QT: 2, QT: 3, P: 2}
 
 
@@ -72,14 +67,13 @@ def tile_rssm_pa_kernel(tc, prev_state, prev_action, obs_bytes, obs_scale, eps,
             xs.append(keep.tile([P, G1, n], U8, name="xs%d" % grp, align_bytes=64))
             hc.append(keep.tile([P, G2, n], U32, name="hc%d" % grp, align_bytes=64))
             hs.append(keep.tile([P, G2, n], U8, name="hs%d" % grp, align_bytes=64))
-        scale_rows = keep.tile([P, P], F32)
-        scale_cols = keep.tile([P, SCALE_ROWS], F32)
-        scale = keep.tile([P, O], F32)
+        scale_mixed = keep.tile([P, 4], F32)
+        scale_obs = keep.tile([P, G1 - STATE_PASSES - 1, 4], F32)
+        ones = keep.tile([ACTION_ROWS, 4], F32)
         b1_cols = keep.tile([P, G2, 4], BF16)
         b2_rows = keep.tile([P, 2 * L], BF16)
         eps_sb = keep.tile([P, NT, L], BF16)
         ident = keep.tile([P, P], F32)
-        ident_bf = keep.tile([P, P], BF16)
 
         raw, woven, rows, obs, banks, hidden, result = {}, {}, {}, {}, {}, {}, {}
         copy = {"vector": nc.vector.tensor_copy, "scalar": nc.scalar.copy}
@@ -87,9 +81,13 @@ def tile_rssm_pa_kernel(tc, prev_state, prev_action, obs_bytes, obs_scale, eps,
         def streamed(tag, shape, dtype):
             return stream.tile(shape, dtype, name=tag, bufs=DEPTH[tag], align_bytes=64)
 
-        def load_scale():
-            nc.sync.dma_start(out=scale_rows[:SCALE_ROWS, :SCALE_COLS],
-                              in_=obs_scale.rearrange("o (r c) -> (o r) c", c=SCALE_COLS))
+        def load_scales():
+            first = KP - A
+            flat = obs_scale.rearrange("o k -> (o k)")
+            nc.sync.dma_start(out=scale_obs[:], in_=flat[first:].rearrange("(g p t) -> p g t", p=P, t=4))
+            mixed = flat[:first].rearrange("(p t) -> p t", t=4)
+            for p0, p1 in ((ACTION_ROWS, P // 2), (P // 2, P)):
+                nc.sync.dma_start(out=scale_mixed[p0:p1, :], in_=mixed[p0 - ACTION_ROWS:p1 - ACTION_ROWS, :])
 
         def load_w1(half, g):
             raw[half, g] = streamed("wraw", [P, 4, KP], BF16)
@@ -100,31 +98,31 @@ def tile_rssm_pa_kernel(tc, prev_state, prev_action, obs_bytes, obs_scale, eps,
             raw[piece] = streamed("wraw", [P, 4, n], BF16)
             nc.sync.dma_start(out=raw[piece][:], in_=w2_v[g][:, :, c0:c0 + n])
 
-        def passes_in_tile(q):
-            return 1 if q in GROUPS[0] else 2
-
-        def rows_depth(q):
-            return 2 if q in GROUPS[0] else 1
-
-        def row_tile(q, g):
-            if (q, g) not in rows:
-                n = passes_in_tile(q)
-                buf = stream.tile([P, 2, n * KP], BF16, name=("rows%d" if n == 1 else "wide%d") % g, bufs=rows_depth(q), align_bytes=64)
-                rows[q, g, "tile"] = buf
-                for j in range(n):
-                    rows[q, g + j] = buf[:, :, KP * j:KP * j + KP]
-            return rows[q, g, "tile"]
-
         def load_state(q, g):
-            k1 = KP * (g + passes_in_tile(q))
-            nc.sync.dma_start(out=row_tile(q, g)[:], in_=state_v[:, 2 * q:2 * q + 2, KP * g:k1])
+            n = 1 if q in GROUPS[0] else STATE_PASSES
+            buf = streamed("state%d" % n, [P, 2, n * KP], BF16)
+            for i in range(2):
+                for j in range(n):
+                    rows[2 * q + i, g + j] = buf[:, i, KP * j:KP * j + KP]
+            nc.sync.dma_start(out=buf[:], in_=state_v[:, 2 * q:2 * q + 2, KP * g:KP * (g + n)])
 
-        def load_action(q):
-            nc.sync.dma_start(out=row_tile(q, STATE_PASSES)[:, :, :A], in_=action_v[:, 2 * q:2 * q + 2, :])
+        def obs_cols(g):
+            return max(KP * g - S - A, 0), KP * (g + 2) - S - A
 
-        def load_obs(q):
-            obs[q] = keep.tile([P, 2, O], U8, name="obs%d" % q)
-            nc.sync.dma_start(out=obs[q][:], in_=bytes_v[:, 2 * q:2 * q + 2, :])
+        def load_obs(q, g):
+            c0, c1 = obs_cols(g)
+            obs[q, g] = streamed("obs%d" % g, [P, 2, c1 - c0], U8)
+            nc.sync.dma_start(out=obs[q, g][:], in_=bytes_v[:, 2 * q:2 * q + 2, c0:c1])
+
+        def wide_tile(n, g):
+            if (n, g) not in rows:
+                buf = streamed("wide%d" % g, [P, 2 * KP], BF16)
+                rows[n, g, "tile"] = buf
+                rows[n, g], rows[n, g + 1] = buf[:, :KP], buf[:, KP:]
+            return rows[n, g, "tile"]
+
+        def load_action(n):
+            nc.sync.dma_start(out=wide_tile(n, STATE_PASSES)[:, :A], in_=action_v[:, n, :])
 
         def load_b1():
             nc.sync.dma_start(out=b1_cols[:], in_=b1.rearrange("(g p t) -> p g t", p=P, t=4))
@@ -135,101 +133,73 @@ def tile_rssm_pa_kernel(tc, prev_state, prev_action, obs_bytes, obs_scale, eps,
         def load_eps():
             nc.sync.dma_start(out=eps_sb[:], in_=eps_v)
 
-        def turn_scale():
-            banks["scale"] = psum.tile([P, P], F32, name="tp")
-            nc.tensor.transpose(banks["scale"][:], scale_rows[:], ident[:])
-
-        def drain_scale():
-            nc.scalar.copy(out=scale_cols[:], in_=banks["scale"][:, :SCALE_ROWS])
-
-        def spread_scale(n):
-            banks["scale", n] = psum.tile([P, 4, P], F32, name="acc")
-            for r in range(4):
-                column = scale_cols[:, 4 * n + r:4 * n + r + 1]
-                nc.tensor.transpose(banks["scale", n][:, r, :], column.to_broadcast([P, P]), ident[:])
-
-        def drain_spread(n):
-            out = scale[:, 4 * SCALE_COLS * n:4 * SCALE_COLS * (n + 1)].rearrange("p (r c) -> p r c", r=4)
-            nc.scalar.copy(out=out, in_=banks["scale", n][:, :, :SCALE_COLS])
-
-        def product(q, g, tiles):
-            k0 = max(KP * g, S + A)
-            c0, c1 = k0 - (S + A), KP * (g + passes_in_tile(q)) - (S + A)
-            for i in tiles:
-                nc.vector.tensor_tensor(out=row_tile(q, g)[:, i, k0 - KP * g:], in0=obs[q][:, i, c0:c1].bitcast(FP8),
-                                        in1=scale[:, c0:c1], op=ALU.mult)
-
-        def product_steps(q, g):
-            return [(product, q, g, (0, 1))] if q in GROUPS[0] else [(product, q, g, (i,)) for i in range(2)]
-
-        def turn_tag(q, g):
-            return "acc" if pair_of(q, g) == LAST_X[2] else "tp"
+        def widen(n, g, engine):
+            c0, c1 = obs_cols(g)
+            copy[engine](out=wide_tile(n, g)[:, 2 * KP - (c1 - c0):], in_=obs[n // 2, g][:, n % 2, :].bitcast(FP8))
 
         def turn(q, g):
             banks[q, g] = psum.tile([P, 2, QT], F32, name=turn_tag(q, g))
             for i in range(2):
-                words = rows[q, g][:, i, :].bitcast(F32)
+                words = rows[2 * q + i, g].bitcast(F32)
                 for u in range(2):
                     nc.tensor.transpose(banks[q, g][:, u, P * i:P * i + P], words[:, u::2], ident[:])
 
-        def bank_pair(n):
-            return [(0, n), (1, n)] if n < G1 else [(n // 3, 2 * (n % 3)), (n // 3, 2 * (n % 3) + 1)]
-
         def pair_of(q, g):
-            return g if q in GROUPS[0] else 3 * q + g // 2
+            return (("front", g), q) if q in GROUPS[0] else ((q, g - g % 2), g % 2)
 
-        def drain_x(n):
-            woven["x", n] = streamed("woven_s", [P, WOVEN], BF16)
-            for j, key in enumerate(bank_pair(n)):
-                out = woven["x", n][:].bitcast(F32)[:, KP * j:KP * j + KP].rearrange("p (r u) -> p r u", u=2)
-                nc.scalar.copy(out=out, in_=banks[key][:].rearrange("p u r -> p r u"))
+        def banks_of(pair):
+            return [(q, pair[1]) for q in GROUPS[0]] if pair[0] == "front" else [pair, (pair[0], pair[1] + 1)]
 
-        def quant_x(n):
-            g0, (q, g1) = bank_pair(n)[0][1], bank_pair(n)[1]
-            grp = max(q - 1, 0)
-            nc.vector.quantize_mx(out=xc[grp][:, g0:g1 + 1, :].rearrange("p g n -> p (g n)").bitcast(FP8X4),
-                                  scales=xs[grp][:, g0:g1 + 1, :].rearrange("p g n -> p (g n)"), in_=woven["x", n][:])
+        def x_half(q, g):
+            pair, j = pair_of(q, g)
+            if ("x", pair) not in woven:
+                woven["x", pair] = streamed("woven_x", [P, WOVEN], BF16)
+            return woven["x", pair][:, WOVEN // 2 * j:WOVEN // 2 * (j + 1)]
 
-        def w1_shares(half, g):
-            cut = RUNS if (half, g) == (0, 0) else VECTOR_RUNS[half]
-            return {"vector": slice(0, cut), "scalar": slice(cut, RUNS)}
+        def drain(q, g):
+            out = x_half(q, g).bitcast(F32).rearrange("p (r u) -> p r u", u=2)
+            nc.scalar.copy(out=out, in_=banks[q, g][:].rearrange("p u r -> p r u"))
 
-        def w1_weavers(half, g, by_tensor):
-            if (half, g) == VIA_TENSOR:
-                return [(by_tensor, half, g, k) for k in range(2)]
-            return [(weave_w1, half, g, e) for e, part in w1_shares(half, g).items() if part.stop > part.start]
+        def product(q, g):
+            scale = scale_mixed[:] if g == STATE_PASSES else scale_obs[:, g - STATE_PASSES - 1, :]
+            nc.vector.tensor_tensor(out=x_half(q, g).rearrange("p (r u e) -> p r u e", u=2, e=2),
+                                    in0=banks[q, g][:].bitcast(BF16).rearrange("p u (r e) -> p r u e", e=2),
+                                    in1=scale.rearrange("p (u e) -> p u e", e=2).unsqueeze(1).to_broadcast([P, QT, 2, 2]),
+                                    op=ALU.mult)
 
-        def weave_w1(half, g, engine):
-            if (half, g) not in woven:
-                woven[half, g] = streamed("woven_w", [P, WOVEN], BF16)
-            part = w1_shares(half, g)[engine]
-            copy[engine](out=woven[half, g][:].rearrange("p (s r e t) -> p r t e s", s=4, e=2, t=4)[:, part],
-                         in_=raw[half, g][:].rearrange("p t (r e s) -> p r t e s", e=2, s=4)[:, part])
+        def quant_x(pair):
+            grp, g0, n = (0, pair[1], 1) if pair[0] == "front" else (pair[0] - 1, pair[1], 2)
+            nc.vector.quantize_mx(out=xc[grp][:, g0:g0 + n, :].rearrange("p g n -> p (g n)").bitcast(FP8X4),
+                                  scales=xs[grp][:, g0:g0 + n, :].rearrange("p g n -> p (g n)"), in_=woven["x", pair][:])
 
-        def pass_w1(half, g, k):
-            banks["w", half, g, k] = psum.tile([P, 2, P, 4], BF16, name="tp")
-            for j in range(2):
-                c0 = 2 * P * k + P * j
-                nc.tensor.matmul(banks["w", half, g, k][:, j], ident_bf[:],
-                                 raw[half, g][:, :, c0:c0 + P].rearrange("p t c -> p c t"), start=True, stop=True)
+        def weave_w1(part, engine, r0, r1):
+            half, g, s0, s1, tag = part
+            if part not in woven:
+                woven[part] = streamed(tag, [P, KP * (s1 - s0)], BF16)
+            if engine == "gpsimd":
+                nc.gpsimd.tensor_scalar(out=woven[part][:].rearrange("p (s m t) -> p s m t", m=P, t=4)[:, :, 2 * r0:2 * r1],
+                                        in0=raw[half, g][:].rearrange("p t (m s) -> p s m t", s=4)[:, s0:s1, 2 * r0:2 * r1],
+                                        scalar1=1.0, scalar2=0.0, op0=ALU.mult, op1=ALU.add)
+            else:
+                copy[engine](out=woven[part][:].rearrange("p (s r e t) -> p r t e s", r=RUNS, e=2, t=4)[:, r0:r1],
+                             in_=raw[half, g][:].rearrange("p t (r e s) -> p r t e s", e=2, s=4)[:, r0:r1, :, :, s0:s1])
 
-        def drain_w1(half, g, k):
-            if k == 0:
-                woven[half, g] = streamed("woven_s", [P, WOVEN], BF16)
-            m0 = 2 * P * k // 4
-            out = woven[half, g][:].bitcast(F32).rearrange("p (s m w) -> p m s w", s=4, w=2)[:, m0:m0 + 2 * P // 4]
-            src = banks["w", half, g, k][:].rearrange("p j c t -> p (j c t)").bitcast(F32)
-            nc.scalar.copy(out=out, in_=src.rearrange("p (m s w) -> p m s w", s=4, w=2))
+        def quant_w1(part):
+            half, g, s0, s1, tag = part
+            cols = slice(KP * half + P * s0, KP * half + P * s1)
+            nc.vector.quantize_mx(out=w1c[:, g, cols].bitcast(FP8X4), scales=w1s[:, g, cols], in_=woven[part][:])
 
-        def quant_w1(half, g):
-            cols = slice(KP * half, KP * half + KP)
-            nc.vector.quantize_mx(out=w1c[:, g, cols].bitcast(FP8X4), scales=w1s[:, g, cols], in_=woven[half, g][:])
+        def weave_tag(engine):
+            return {"vector": "woven_v", "scalar": "woven_s", "gpsimd": "woven_g"}[engine]
 
         def weave(key, src, engine):
-            buf = streamed("woven_v" if engine == "vector" else "woven_s", [P, WOVEN], BF16)
-            woven[key] = buf[:, :4 * src.shape[2]]
-            copy[engine](out=woven[key].rearrange("p (r e t) -> p r t e", e=8, t=4),
-                         in_=src.rearrange("p t (r e) -> p r t e", e=8))
+            woven[key] = streamed(weave_tag(engine), [P, 4 * src.shape[2]], BF16)[:]
+            if engine == "gpsimd":
+                nc.gpsimd.tensor_scalar(out=woven[key].rearrange("p (c t) -> p c t", t=4), in0=src.rearrange("p t c -> p c t"),
+                                        scalar1=1.0, scalar2=0.0, op0=ALU.mult, op1=ALU.add)
+            else:
+                copy[engine](out=woven[key].rearrange("p (r e t) -> p r t e", e=8, t=4),
+                             in_=src.rearrange("p t (r e) -> p r t e", e=8))
 
         def weave_w2(piece, engine):
             weave(piece, raw[piece][:], engine)
@@ -243,17 +213,14 @@ def tile_rssm_pa_kernel(tc, prev_state, prev_action, obs_bytes, obs_scale, eps,
             cols = slice(KP * half + P * t, KP * half + P * t + P)
             nc.tensor.matmul_mx(out=banks[span, half, t], lhsT=w1c[:, g, cols].bitcast(FP8X4), lhsT_scale=w1s[:, g, cols],
                                 rhs=xc[grp][:, g, r0:r0 + n].bitcast(FP8X4), rhs_scale=xs[grp][:, g, r0:r0 + n],
-                                start=(g == 0), stop=(g == G1 - 1))
+                                start=(g == ORDER[0]), stop=(g == ORDER[-1]))
 
         def front_pass(half, g):
             for t in range(4):
-                if g == 0:
+                if g == ORDER[0]:
                     acc = psum.tile([P, KP], F32, name="acc")
                     banks[FRONT, half, t] = acc[:]
                 mm1(FRONT, half, t, g)
-
-        def bank_tag(span, half):
-            return "tp" if (span, half) == (THIRD, 0) else "acc"
 
         def bank_start(span, t):
             return t - t % (KP // span[2])
@@ -263,7 +230,7 @@ def tile_rssm_pa_kernel(tc, prev_state, prev_action, obs_bytes, obs_scale, eps,
             acc = psum.tile([P, KP // n, n], F32, name=bank_tag(span, half))
             for t in range(t0, t0 + KP // n):
                 banks[span, half, t] = acc[:, t - t0, :]
-                for g in range(G1):
+                for g in ORDER:
                     mm1(span, half, t, g)
 
         def relu(span, half, t0):
@@ -325,99 +292,137 @@ def tile_rssm_pa_kernel(tc, prev_state, prev_action, obs_bytes, obs_scale, eps,
         def store_sample(n, c0=0, c1=L):
             nc.sync.dma_start(out=sample_v[:, n, c0:c1], in_=result[n, "sample"][:, c0:c1])
 
-        def rows_of(q):
-            return [(load_obs, q), (load_state, q, 0), (load_action, q)]
+        def turn_tag(q, g):
+            return "tp"
 
-        def turns(n):
-            return [(turn, q, g) for q, g in bank_pair(n)]
+        def bank_tag(span, half):
+            return "tp" if (span, half) == (THIRD, 0) else "acc"
+
+        def turns(pair):
+            return [(turn, q, g) for q, g in banks_of(pair)]
+
+        def empties(pair):
+            return [(drain if g < STATE_PASSES else product, q, g) for q, g in banks_of(pair)]
 
         def relus(span, half):
             return [(relu, span, half, 0), (relu, span, half, 2)]
 
-        sync_q = [(load_scale,), (load_w1, 0, 0), (load_obs, 0), (load_obs, 1), (load_w1, 0, 1)]
-        sync_q += [(load_state, q, g) for g in range(STATE_PASSES) for q in GROUPS[0]]
-        sync_q += [(load_action, q) for q in GROUPS[0]] + [(load_w1, 0, g) for g in range(2, G1)] + [(load_b1,)]
-        sync_q += rows_of(2) + [(load_w1, 1, g) for g in range(G1)] + rows_of(3)
-        sync_q += [(load_w2, piece) for piece in W2_PIECES] + [(load_b2,), (load_eps,)]
-        for n in range(NT):
-            sync_q += [(store_std, n), (store_mean, n)] + ([(store_sample, n - 1)] if n else [])
+        def front(g):
+            return ("front", g)
+
+        def whole(half, g):
+            return (half, g, 0, 4, "woven_w")
+
+        def low(half, g):
+            return (half, g, 0, 2, "woven_g")
+
+        def high(half, g):
+            return (half, g, 2, 4, "woven_w")
+
+        def by(engine, part, r0=0, r1=RUNS):
+            return (weave_w1, part, engine, r0, r1)
+
+        def rows_of(q):
+            return [(load_obs, q, 4), (load_state, q, 0), (load_obs, q, 2), (load_action, 2 * q), (load_action, 2 * q + 1)]
+
+        def widens(q, g):
+            return [(widen, 2 * q, g, "scalar"), (widen, 2 * q + 1, g, "scalar")]
+
         halves = [(NT - 1, 0, L // 2), (NT - 1, L // 2, L)]
-        sync_q += [(store_sample,) + part for part in halves]
-
-        tensor_q = [(turn_scale,)] + [(spread_scale, n) for n in range(SCALE_ROWS // 4)]
-        for n in range(LEAD):
-            tensor_q += turns(n)
-        for g in range(G1):
-            tensor_q += [(front_pass, 0, g)] + (w1_weavers(*VIA_TENSOR, pass_w1) if g == G1 - 1 else [])
-            tensor_q += turns(g + LEAD)
-        tensor_q += [(front_pass, 1, 0), (fill_bank, THIRD, 0, 0), (fill_bank, THIRD, 0, 2)]
-        tensor_q += [(front_pass, 1, g) for g in range(1, G1)]
-        tensor_q += turns(LAST_X[0]) + [(fill_bank, THIRD, 1, 0)] + turns(LAST_X[1])
-        tensor_q += [(fill_bank, THIRD, 1, 2)] + turns(LAST_X[2]) + [(heads, 0), (heads, 1)]
-        for n, bank in enumerate(((LAST, 0, 0), (LAST, 0, 2), (LAST_A, 1, 0), (LAST_B, 1, 0))):
-            tensor_q += [(heads, n + 2), (fill_bank,) + bank]
-        tensor_q += [(heads, NT - 2), (heads, NT - 1, FIRST_PASS), (heads, NT - 1, SECOND_PASS)]
-
-        scalar_q = [(drain_scale,)] + [(drain_spread, n) for n in range(SCALE_ROWS // 4)]
-        scalar_q += [(weave_w1, 0, 1, "scalar"), (drain_x, 0), (drain_x, 1)]
-        for g in range(2, G1):
-            scalar_q += [(weave_w1, 0, g, "scalar"), (drain_x, g)]
-        scalar_q += [(drain_x, THIRD_X[0]), (weave_w1, 1, 0, "scalar"), (drain_x, THIRD_X[1])]
-        scalar_q += relus(FRONT, 0) + [(drain_x, THIRD_X[2])]
-        scalar_q += w1_weavers(*VIA_TENSOR, drain_w1) + [(weave_w1, 1, g, "scalar") for g in range(2, G1)]
-        scalar_q += relus(THIRD, 0)
-        scalar_q += [(weave_w2, W2_PIECES[0], "scalar")] + relus(FRONT, 1) + [(weave_h, FRONT, 1, "scalar")]
-        scalar_q += [(drain_x, n) for n in LAST_X] + relus(THIRD, 1)
-        after_root = [[(weave_h, THIRD, 0, "scalar")], [(weave_h, THIRD, 1, "scalar")], [(relu, LAST, 0, 0)],
-                      [(relu, LAST, 0, 2), (weave_h, LAST, 0, "scalar")],
-                      relus(LAST_A, 1) + [(weave_h, LAST_A, 1, "scalar")], relus(LAST_B, 1), [], []]
+        stores = []
         for n in range(NT):
-            scalar_q += [(root, n)] + after_root[n]
+            stores += [(store_std, n), (store_mean, n)] + ([(store_sample, n - 1)] if n else [])
+        stores += [(store_sample,) + part for part in halves]
 
-        products = [step for g in range(STATE_PASSES, G1) for q in GROUPS[0] for step in product_steps(q, g)]
-        products += [step for q in (2, 3) for g in range(STATE_PASSES, G1, 2) for step in product_steps(q, g)]
-        vector_q = [(weave_w1, 0, 0, "vector"), products.pop(0), (quant_w1, 0, 0), products.pop(0), products.pop(0)]
-        vector_q += [(weave_w1, 0, 1, "vector"), products.pop(0), (quant_w1, 0, 1), (quant_x, 0), (quant_x, 1)]
-        for g in range(2, G1):
-            vector_q += [(weave_w1, 0, g, "vector"), products.pop(0), (quant_w1, 0, g)]
-            vector_q += ([products.pop(0)] if g + STATE_PASSES < G1 else []) + [(quant_x, g)]
-        vector_q += [(weave_w1, 1, 0, "vector"), products.pop(0), (quant_w1, 1, 0), products.pop(0)]
-        vector_q += [(quant_x, THIRD_X[0]), (quant_x, THIRD_X[1]), (weave_w1, 1, 2, "vector")]
-        vector_q += [(quant_x, THIRD_X[2]), products.pop(0)]
-        for g in range(1, G1):
-            vector_q += [(quant_w1, 1, g), (weave_w1, 1, g + 2, "vector") if g + 2 < G1 else products.pop(0)]
-        vector_q += [(weave_h, FRONT, 0, "vector"), products.pop(0), (quant_h, FRONT, 0)]
-        w2_order = W2_PIECES[0::2] + W2_PIECES[1::2]
-        for piece, following in zip(w2_order, w2_order[1:]):
-            vector_q += [(weave_w2, following, "vector"), (quant_w2, piece)]
-        vector_q += [(quant_w2, w2_order[-1]), (quant_h, FRONT, 1), (quant_x, LAST_X[0]), (quant_x, LAST_X[1])]
-        after_tile = [[(quant_x, LAST_X[2])], [], [(quant_h, THIRD, 0), (quant_h, THIRD, 1)], [],
-                      [(quant_h, LAST, 0)], [(quant_h, LAST_A, 1)]]
-        for n in range(NT - 2):
+        first, second = (0, 4, 0, 4, "woven_g"), (1, 5, 0, 4, "woven_g")
+        sync_q = [(load_obs, 0, 4), (load_w1, 0, 4), (load_scales,), (load_obs, 1, 4), (load_w1, 0, 5), (load_state, 0, 0), (load_state, 1, 0)]
+        for q in GROUPS[0]:
+            sync_q += [(load_obs, q, 2), (load_action, 2 * q), (load_action, 2 * q + 1)]
+        sync_q += [(load_w1, 0, 0), (load_w1, 0, 2), (load_state, 0, 1), (load_state, 1, 1), (load_w1, 0, 1), (load_w1, 0, 3), (load_b1,)]
+        sync_q += rows_of(2) + [(load_w1, 1, g) for g in (4, 5, 0, 3, 2, 1)] + rows_of(3)
+        sync_q += [(load_w2, piece) for piece in W2_PIECES] + [(load_b2,), (load_eps,)] + stores
+
+        tensor_q = [(turn, q, g) for q in GROUPS[0] for g in (4, 5)] + turns(front(0)) + turns(front(2)) + [(front_pass, 0, 4)]
+        tensor_q += turns(front(1)) + [(front_pass, 0, 5)] + turns(front(3)) + [(front_pass, 0, 0), (front_pass, 0, 2)]
+        tensor_q += turns((2, 4)) + [(front_pass, 0, 1)] + turns((2, 0)) + [(front_pass, 0, 3)] + turns((2, 2))
+        tensor_q += [(front_pass, 1, 4), (front_pass, 1, 5)] + turns((3, 4)) + [(front_pass, 1, 0), (fill_bank, THIRD, 0, 0)]
+        tensor_q += [(front_pass, 1, 2), (front_pass, 1, 1), (front_pass, 1, 3), (fill_bank, THIRD, 0, 2)] + turns((3, 2))
+        tensor_q += [(fill_bank, THIRD, 1, 0)] + turns((3, 0)) + [(fill_bank, THIRD, 1, 2), (heads, 0), (heads, 1)]
+
+        gpsimd_q = [by("gpsimd", low(0, g)) for g in (5, 2, 3)] + [by("gpsimd", low(1, g)) for g in (4, 3)]
+        gpsimd_q += [(weave_w2, W2_PIECES[1], "gpsimd"), (weave_w2, W2_PIECES[3], "gpsimd")]
+
+        scalar_q = widens(0, 4) + widens(1, 4) + [by("scalar", high(0, 5))] + widens(0, 2) + [(drain, 0, 0)] + widens(1, 2) + [(drain, 1, 0)]
+        scalar_q += [by("scalar", whole(0, 0)), by("scalar", high(0, 2))] + empties(front(1)) + [by("scalar", whole(0, 1))]
+        scalar_q += widens(2, 4) + [by("scalar", high(0, 3)), by("scalar", high(1, 4))] + widens(2, 2) + empties((2, 0))
+        scalar_q += relus(FRONT, 0) + [by("scalar", whole(1, 0))] + widens(3, 4)
+        scalar_q += [by("scalar", whole(1, 2)), by("scalar", high(1, 3))] + widens(3, 2) + [(relu, THIRD, 0, 0)]
+        scalar_q += [(weave_w2, W2_PIECES[0], "scalar")] + relus(FRONT, 1) + [(relu, THIRD, 0, 2)]
+        scalar_q += [(weave_h, FRONT, 1, "scalar")] + empties((3, 0)) + relus(THIRD, 1)
+
+        vector_q = [by("vector", first), (product, 0, 4), (product, 0, 5), (quant_w1, first), (product, 1, 4), (product, 1, 5)]
+        vector_q += [(quant_w1, high(0, 5)), (quant_x, front(4)), (quant_x, front(5)), (quant_x, front(0)), (quant_w1, low(0, 5))]
+        vector_q += empties(front(2)) + [(quant_w1, whole(0, 0)), (quant_x, front(2)), (quant_w1, high(0, 2)), (quant_x, front(1)), (quant_w1, low(0, 2))]
+        vector_q += empties(front(3)) + [(quant_w1, whole(0, 1)), (quant_x, front(3)), (quant_w1, high(0, 3)), (quant_w1, low(0, 3))]
+        vector_q += empties((2, 4)) + [(quant_w1, high(1, 4)), (quant_w1, low(1, 4)), by("vector", second), (quant_x, (2, 4)), (quant_w1, second)]
+        vector_q += empties((2, 2)) + [(quant_w1, whole(1, 0)), (quant_x, (2, 2)), (quant_x, (2, 0)), by("vector", whole(1, 1))]
+        vector_q += [(quant_w1, whole(1, 2)), (quant_w1, whole(1, 1)), (quant_w1, high(1, 3)), (quant_w1, low(1, 3))]
+        vector_q += empties((3, 4)) + [(weave_h, FRONT, 0, "vector"), (quant_x, (3, 4)), (quant_h, FRONT, 0)]
+        vector_q += [(weave_w2, W2_PIECES[2], "vector"), (quant_w2, W2_PIECES[1])] + empties((3, 2))
+        vector_q += [(quant_w2, W2_PIECES[2]), (quant_w2, W2_PIECES[0]), (quant_x, (3, 2))]
+        vector_q += [(quant_w2, W2_PIECES[3]), (quant_h, FRONT, 1), (quant_x, (3, 0))]
+
+        after_root = [[(weave_h, THIRD, 0, "scalar")], [(relu, LAST, 0, 0), (weave_h, THIRD, 1, "scalar")],
+                      [(relu, LAST, 0, 2), (weave_h, LAST, 0, "scalar")],
+                      relus(LAST_A, 1) + [(weave_h, LAST_A, 1, "scalar")], [], [], [], []]
+        for n in range(NT):
+            scalar_q += (relus(LAST_B, 1) if n == 5 else []) + [(root, n)] + after_root[n]
+        after_tile = [[], [(quant_h, THIRD, 0)], [(quant_h, THIRD, 1)], [(quant_h, LAST, 0)], [(quant_h, LAST_A, 1)]]
+        for n in range(NT - 3):
             vector_q += [(bias_wide, n)] + ([(noise, n - 1)] if n else []) + [(bias_narrow, n)]
             vector_q += ([(shift, n - 1)] if n else []) + after_tile[n]
-        vector_q += [(noise, 5), (weave_h, LAST_B, 1, "vector"), (shift, 5), (quant_h, LAST_B, 1)]
-        vector_q += [(bias_wide, 6), (bias_narrow, 6), (bias_wide, 7), (noise, 6), (bias_narrow, 7), (shift, 6)]
+        vector_q += [(bias_wide, 5), (noise, 4), (bias_narrow, 5), (shift, 4), (weave_h, LAST_B, 1, "vector"), (bias_wide, 6), (quant_h, LAST_B, 1)]
+        vector_q += [(noise, 5), (bias_narrow, 6), (shift, 5), (bias_wide, 7), (noise, 6), (bias_narrow, 7), (shift, 6)]
         vector_q += [(f,) + part for f in (noise, shift) for part in halves]
+        tensor_q += [(fill_bank, LAST, 0, 0), (heads, 2), (fill_bank, LAST, 0, 2), (heads, 3), (fill_bank, LAST_A, 1, 0), (heads, 4), (heads, 5)]
+        tensor_q += [(fill_bank, LAST_B, 1, 0), (heads, NT - 2), (heads, NT - 1, FIRST_PASS), (heads, NT - 1, SECOND_PASS)]
+        behind = {by("gpsimd", low(1, 3)): [(quant_w1, second)]}
 
-        weaver = {step[1:-1]: step for step in vector_q + scalar_q if step[0] in (weave_w2, weave_h)}
+        everything = sync_q + tensor_q + scalar_q + vector_q + gpsimd_q
+        weaver = {step[1:-1]: step for step in everything if step[0] in (weave_w2, weave_h)}
+        widener = {step[1:-1]: step for step in everything if step[0] == widen}
+
+        def w1_steps(f, half, g):
+            return [step for step in everything if step[0] == f and step[1][:2] == (half, g)]
+
+        def emptier(q, g):
+            return (drain if g < STATE_PASSES else product, q, g)
 
         def needs(f, *a):
-            if f == product:
-                return [(load_obs, a[0])] + [(drain_spread, n) for n in range(a[1] - 1)]
+            if f == widen:
+                return [(load_obs, a[0] // 2, a[1])]
             if f == turn:
-                q, g = a[0], a[1] - a[1] % passes_in_tile(a[0])
-                return [(load_state, q, g)] if g < STATE_PASSES else product_steps(q, g) + [(load_action, q)]
+                q, g = a
+                if g < STATE_PASSES:
+                    return [(load_state, q, g if q in GROUPS[0] else 0)]
+                tiles = (2 * q, 2 * q + 1)
+                return [widener[n, g - g % 2] for n in tiles] + [(load_action, n) for n in tiles if g < STATE_PASSES + 2]
+            if f == product:
+                return [(turn,) + a, (load_scales,)]
+            if f == quant_x:
+                return [emptier(*key) for key in banks_of(a[0])]
+            if f == weave_w1:
+                return [(load_w1,) + a[0][:2]]
             if f == quant_w1:
-                return w1_weavers(a[0], a[1], drain_w1)
+                return [step for step in everything if step[0] == weave_w1 and step[1] == a[0]]
             if f == front_pass:
-                return [(quant_w1,) + a, (quant_x, a[1])]
+                return w1_steps(quant_w1, *a) + [(quant_x, ("front", a[1]))]
             if f == fill_bank:
                 quarter = GROUPS[a[0][0]][0]
-                return [(quant_w1, a[1], g) for g in range(G1)] + [(quant_x, pair_of(quarter, g)) for g in range(G1)]
+                return [s for g in ORDER for s in w1_steps(quant_w1, a[1], g) + [(quant_x, pair_of(quarter, g)[0])]]
             if f == relu:
                 span, half, t0 = a
-                sums = (front_pass, half, G1 - 1) if span == FRONT else (fill_bank, span, half, bank_start(span, t0))
+                sums = (front_pass, half, ORDER[-1]) if span == FRONT else (fill_bank, span, half, bank_start(span, t0))
                 return [(load_b1,), sums]
             if f == heads:
                 passes = a[1] if len(a) > 1 else ALL_PASSES
@@ -425,68 +430,63 @@ def tile_rssm_pa_kernel(tc, prev_state, prev_action, obs_bytes, obs_scale, eps,
                 return pieces + [(quant_w2, piece) for piece in W2_PIECES]
             if f == bias_wide:
                 return [(heads, a[0], SECOND_PASS) if a[0] == NT - 1 else (heads, a[0]), (load_b2,)]
-            if f == drain_x:
-                return turns(a[0])
             if f == weave_h:
                 return relus(a[0], a[1])
             if f in (quant_w2, quant_h):
                 return [weaver[a]]
-            simple = {turn_scale: [(load_scale,)], drain_scale: [(turn_scale,)], spread_scale: [(drain_scale,)],
-                      drain_spread: [(spread_scale,) + a], quant_x: [(drain_x,) + a],
-                      weave_w1: [(load_w1,) + a[:2]], pass_w1: [(load_w1,) + a[:2]], drain_w1: [(pass_w1,) + a],
-                      weave_w2: [(load_w2,) + a[:1]], bias_narrow: [(bias_wide,) + a], root: [(bias_wide,) + a],
-                      noise: [(root,) + a[:1], (load_eps,)], shift: [(noise,) + a, (bias_narrow,) + a[:1]],
-                      store_std: [(bias_wide,) + a], store_mean: [(bias_narrow,) + a], store_sample: [(shift,) + a]}
+            simple = {drain: [(turn,) + a], weave_w2: [(load_w2,) + a[:1]], bias_narrow: [(bias_wide,) + a],
+                      root: [(bias_wide,) + a], noise: [(root,) + a[:1], (load_eps,)],
+                      shift: [(noise,) + a, (bias_narrow,) + a[:1]], store_std: [(bias_wide,) + a],
+                      store_mean: [(bias_narrow,) + a], store_sample: [(shift,) + a]}
             return simple.get(f, [])
 
         def takes(f, *a):
             if f == load_w1:
-                return [("wraw", DEPTH["wraw"], w1_weavers(a[0], a[1], pass_w1))]
+                return [("wraw", DEPTH["wraw"], w1_steps(weave_w1, *a))]
             if f == load_w2:
                 return [("wraw", DEPTH["wraw"], [weaver[a]])]
-            if f in (load_state, load_action, product):
-                q, g = a[:2] if f != load_action else (a[0], STATE_PASSES)
-                n = passes_in_tile(q)
-                return [] if (q, g) in rows else [(("rows", n, g), rows_depth(q), [(turn, q, g + j) for j in range(n)])]
+            if f == load_obs:
+                return [("obs%d" % a[1], DEPTH["obs%d" % a[1]], [widener[2 * a[0] + i, a[1]] for i in range(2)])]
+            if f == load_state:
+                n = 1 if a[0] in GROUPS[0] else STATE_PASSES
+                return [("state%d" % n, DEPTH["state%d" % n], [(turn, a[0], a[1] + j) for j in range(n)])]
+            if f in (load_action, widen):
+                n, g = a[0], a[1] if f == widen else STATE_PASSES
+                tag = "wide%d" % g
+                return [] if (n, g) in rows else [(tag, DEPTH[tag], [(turn, n // 2, g), (turn, n // 2, g + 1)])]
             if f == weave_w1:
-                return [] if a[:2] in woven else [("woven_w", DEPTH["woven_w"], [(quant_w1,) + a[:2]])]
+                return [] if a[0] in woven else [(a[0][4], DEPTH[a[0][4]], [(quant_w1, a[0])])]
             if f in (weave_w2, weave_h):
-                tag = "woven_v" if a[-1] == "vector" else "woven_s"
+                tag = weave_tag(a[-1])
                 return [(tag, DEPTH[tag], [(quant_w2 if f == weave_w2 else quant_h,) + a[:-1]])]
-            if f == pass_w1:
-                return [("tp", DEPTH["tp"], [(drain_w1,) + a])]
-            if f == drain_w1 and a[2] == 0:
-                return [("woven_s", DEPTH["woven_s"], [(quant_w1,) + a[:2]])]
-            if f == drain_x:
-                return [("woven_s", DEPTH["woven_s"], [(quant_x,) + a])]
-            if f == turn_scale:
-                return [("tp", DEPTH["tp"], [(drain_scale,)])]
-            if f == spread_scale:
-                return [("acc", DEPTH["acc"], [(drain_spread,) + a])]
+            if f in (drain, product):
+                pair = pair_of(*a)[0]
+                return [] if ("x", pair) in woven else [("woven_x", DEPTH["woven_x"], [(quant_x, pair)])]
             if f == turn:
-                return [(turn_tag(*a), DEPTH["tp"], [(drain_x, pair_of(*a))])]
-            if f == front_pass and a[1] == 0:
-                return [("acc", DEPTH["acc"], [(relu, FRONT, a[0], t - t % 2)]) for t in range(4)]
+                return [(turn_tag(*a), 4, [emptier(*a)])]
+            if f == front_pass and a[1] == ORDER[0]:
+                return [("acc", 4, [(relu, FRONT, a[0], t - t % 2)]) for t in range(4)]
             if f == fill_bank:
-                return [(bank_tag(a[0], a[1]), DEPTH["acc"], [(relu, a[0], a[1], a[2] + KP // a[0][2] - 2)])]
+                return [(bank_tag(a[0], a[1]), 4, [(relu, a[0], a[1], a[2] + KP // a[0][2] - 2)])]
             if f == relu and a[2] == 0:
                 return [(("hidden", a[0][2]), HIDDEN_DEPTH[a[0][2]], [weaver[a[:2]]])]
             if f == heads and a[1:] != (SECOND_PASS,):
-                return [("tp", DEPTH["tp"], [(bias_wide, a[0])]), ("tp", DEPTH["tp"], [(bias_narrow, a[0])])]
+                return [("tp", 4, [(bias_wide, a[0])]), ("tp", 4, [(bias_narrow, a[0])])]
             if f == bias_wide:
-                return [("res", DEPTH["res"], [(store_std,) + a, (store_mean,) + a, (store_sample,) + a])]
+                stores = [s for s in sync_q if s[0] in (store_std, store_mean, store_sample) and s[1] == a[0]]
+                return [("res", DEPTH["res"], stores)]
             return []
 
-        nc.gpsimd.memset(scale_rows[:], 0.0)
+        nc.vector.memset(ones[:], 1.0)
         make_identity(nc, ident[:])
-        nc.scalar.activation(ident_bf[:], ident[:], ACT.Sqrt)
+        nc.scalar.activation(scale_mixed[:ACTION_ROWS, :], ones[:], ACT.Sqrt)
 
         done, held = set(), {}
-        queues = [sync_q, tensor_q, scalar_q, vector_q]
+        queues = [sync_q, tensor_q, scalar_q, vector_q, gpsimd_q]
         while any(queues):
             moved = False
             for queue in queues:
-                if not queue or not all(other in done for other in needs(*queue[0])):
+                if not queue or not all(other in done for other in needs(*queue[0]) + behind.get(queue[0], [])):
                     continue
                 slots = takes(*queue[0])
                 taken = {tag: list(held.get(tag, [])) for tag, depth, readers in slots}

@@ -36,6 +36,7 @@ ORDER = (4, 5, 0, 2, 1, 3)
 DEPTH = {"wraw": 7, "woven_w": 3, "woven_g": 1, "woven_v": 1, "woven_s": 2, "woven_x": 3, "res": 4,
          "state1": 4, "state2": 1, "wide2": 8, "wide4": 4, "obs2": 2, "obs4": 2}
 HIDDEN_DEPTH = {2 * QT: 2, QT: 3, P: 2}
+HEAD_RUNS = 44
 
 
 def tile_rssm_pa_kernel(tc, prev_state, prev_action, obs_bytes, obs_scale, eps,
@@ -172,13 +173,17 @@ def tile_rssm_pa_kernel(tc, prev_state, prev_action, obs_bytes, obs_scale, eps,
             nc.vector.quantize_mx(out=xc[grp][:, g0:g0 + n, :].rearrange("p g n -> p (g n)").bitcast(FP8X4),
                                   scales=xs[grp][:, g0:g0 + n, :].rearrange("p g n -> p (g n)"), in_=woven["x", pair][:])
 
+        def quant_first(q):
+            g, cols = ORDER[0], slice(QT * q, QT * q + QT)
+            nc.vector.quantize_mx(out=xc[0][:, g, cols].bitcast(FP8X4), scales=xs[0][:, g, cols], in_=x_half(q, g))
+
         def weave_w1(part, engine, r0, r1):
             half, g, s0, s1, tag = part
             if part not in woven:
                 woven[part] = streamed(tag, [P, KP * (s1 - s0)], BF16)
             if engine == "gpsimd":
-                nc.gpsimd.tensor_scalar(out=woven[part][:].rearrange("p (s m t) -> p s m t", m=P, t=4)[:, :, 2 * r0:2 * r1],
-                                        in0=raw[half, g][:].rearrange("p t (m s) -> p s m t", s=4)[:, s0:s1, 2 * r0:2 * r1],
+                nc.gpsimd.tensor_scalar(out=woven[part][:].rearrange("p (s m t) -> p m s t", m=P, t=4)[:, 2 * r0:2 * r1],
+                                        in0=raw[half, g][:].rearrange("p t (m s) -> p m s t", s=4)[:, 2 * r0:2 * r1, s0:s1],
                                         scalar1=1.0, scalar2=0.0, op0=ALU.mult, op1=ALU.add)
             else:
                 copy[engine](out=woven[part][:].rearrange("p (s r e t) -> p r t e s", r=RUNS, e=2, t=4)[:, r0:r1],
@@ -210,10 +215,11 @@ def tile_rssm_pa_kernel(tc, prev_state, prev_action, obs_bytes, obs_scale, eps,
 
         def mm1(span, half, t, g):
             grp, r0, n = span
+            sums = banks[FRONT, half, t][:, r0:r0 + n] if grp == 0 else banks[span, half, t]
             cols = slice(KP * half + P * t, KP * half + P * t + P)
-            nc.tensor.matmul_mx(out=banks[span, half, t], lhsT=w1c[:, g, cols].bitcast(FP8X4), lhsT_scale=w1s[:, g, cols],
+            nc.tensor.matmul_mx(out=sums, lhsT=w1c[:, g, cols].bitcast(FP8X4), lhsT_scale=w1s[:, g, cols],
                                 rhs=xc[grp][:, g, r0:r0 + n].bitcast(FP8X4), rhs_scale=xs[grp][:, g, r0:r0 + n],
-                                start=(g == ORDER[0]), stop=(g == ORDER[-1]))
+                                start=(g == ORDER[0] and r0 % KP == 0 or g == ORDER[0] and grp > 0), stop=(g == ORDER[-1]))
 
         def front_pass(half, g):
             for t in range(4):
@@ -221,6 +227,13 @@ def tile_rssm_pa_kernel(tc, prev_state, prev_action, obs_bytes, obs_scale, eps,
                     acc = psum.tile([P, KP], F32, name="acc")
                     banks[FRONT, half, t] = acc[:]
                 mm1(FRONT, half, t, g)
+
+        def first_pass(q):
+            for t in range(4):
+                if q == 0:
+                    acc = psum.tile([P, KP], F32, name="acc")
+                    banks[FRONT, 0, t] = acc[:]
+                mm1((0, QT * q, QT), 0, t, ORDER[0])
 
         def bank_start(span, t):
             return t - t % (KP // span[2])
@@ -339,34 +352,34 @@ def tile_rssm_pa_kernel(tc, prev_state, prev_action, obs_bytes, obs_scale, eps,
         for q in GROUPS[0]:
             sync_q += [(load_obs, q, 2), (load_action, 2 * q), (load_action, 2 * q + 1)]
         sync_q += [(load_w1, 0, 0), (load_w1, 0, 2), (load_state, 0, 1), (load_state, 1, 1), (load_w1, 0, 1), (load_w1, 0, 3), (load_b1,)]
-        sync_q += rows_of(2) + [(load_w1, 1, g) for g in (4, 5, 0, 3, 2, 1)] + rows_of(3)
+        sync_q += rows_of(2) + [(load_w1, 1, g) for g in (4, 5, 0)] + [(load_obs, 3, 4)] + [(load_w1, 1, g) for g in (3, 1, 2)] + rows_of(3)[1:]
         sync_q += [(load_w2, piece) for piece in W2_PIECES] + [(load_b2,), (load_eps,)] + stores
 
         tensor_q = [(turn, q, g) for q in GROUPS[0] for g in (4, 5)] + turns(front(0)) + turns(front(2)) + [(front_pass, 0, 4)]
         tensor_q += turns(front(1)) + [(front_pass, 0, 5)] + turns(front(3)) + [(front_pass, 0, 0), (front_pass, 0, 2)]
-        tensor_q += turns((2, 4)) + [(front_pass, 0, 1)] + turns((2, 0)) + [(front_pass, 0, 3)] + turns((2, 2))
-        tensor_q += [(front_pass, 1, 4), (front_pass, 1, 5)] + turns((3, 4)) + [(front_pass, 1, 0), (fill_bank, THIRD, 0, 0)]
+        tensor_q += turns((2, 4)) + [(front_pass, 0, 1)]
+        tensor_q += [(front_pass, 0, 3)] + turns((2, 2)) + [(front_pass, 1, 4)] + turns((2, 0)) + [(front_pass, 1, 5)] + turns((3, 4)) + [(front_pass, 1, 0), (fill_bank, THIRD, 0, 0)]
         tensor_q += [(front_pass, 1, 2), (front_pass, 1, 1), (front_pass, 1, 3), (fill_bank, THIRD, 0, 2)] + turns((3, 2))
         tensor_q += [(fill_bank, THIRD, 1, 0)] + turns((3, 0)) + [(fill_bank, THIRD, 1, 2), (heads, 0), (heads, 1)]
 
         gpsimd_q = [by("gpsimd", low(0, g)) for g in (5, 2, 3)] + [by("gpsimd", low(1, g)) for g in (4, 3)]
         gpsimd_q += [(weave_w2, W2_PIECES[1], "gpsimd"), (weave_w2, W2_PIECES[3], "gpsimd")]
 
-        scalar_q = widens(0, 4) + widens(1, 4) + [by("scalar", high(0, 5))] + widens(0, 2) + [(drain, 0, 0)] + widens(1, 2) + [(drain, 1, 0)]
+        scalar_q = widens(0, 4) + [by("scalar", first, HEAD_RUNS)] + widens(1, 4) + [by("scalar", high(0, 5))] + widens(0, 2) + [(drain, 0, 0)] + widens(1, 2) + [(drain, 1, 0)]
         scalar_q += [by("scalar", whole(0, 0)), by("scalar", high(0, 2))] + empties(front(1)) + [by("scalar", whole(0, 1))]
-        scalar_q += widens(2, 4) + [by("scalar", high(0, 3)), by("scalar", high(1, 4))] + widens(2, 2) + empties((2, 0))
-        scalar_q += relus(FRONT, 0) + [by("scalar", whole(1, 0))] + widens(3, 4)
+        scalar_q += widens(2, 4) + [by("scalar", high(0, 3)), by("scalar", high(1, 4))] + widens(2, 2)
+        scalar_q += relus(FRONT, 0) + widens(3, 4) + [by("scalar", whole(1, 0))] + empties((2, 0))
         scalar_q += [by("scalar", whole(1, 2)), by("scalar", high(1, 3))] + widens(3, 2) + [(relu, THIRD, 0, 0)]
         scalar_q += [(weave_w2, W2_PIECES[0], "scalar")] + relus(FRONT, 1) + [(relu, THIRD, 0, 2)]
         scalar_q += [(weave_h, FRONT, 1, "scalar")] + empties((3, 0)) + relus(THIRD, 1)
 
-        vector_q = [by("vector", first), (product, 0, 4), (product, 0, 5), (quant_w1, first), (product, 1, 4), (product, 1, 5)]
+        vector_q = [by("vector", first, 0, HEAD_RUNS), (product, 0, 4), (product, 0, 5), (quant_w1, first), (product, 1, 4), (product, 1, 5)]
         vector_q += [(quant_w1, high(0, 5)), (quant_x, front(4)), (quant_x, front(5)), (quant_x, front(0)), (quant_w1, low(0, 5))]
         vector_q += empties(front(2)) + [(quant_w1, whole(0, 0)), (quant_x, front(2)), (quant_w1, high(0, 2)), (quant_x, front(1)), (quant_w1, low(0, 2))]
         vector_q += empties(front(3)) + [(quant_w1, whole(0, 1)), (quant_x, front(3)), (quant_w1, high(0, 3)), (quant_w1, low(0, 3))]
         vector_q += empties((2, 4)) + [(quant_w1, high(1, 4)), (quant_w1, low(1, 4)), by("vector", second), (quant_x, (2, 4)), (quant_w1, second)]
-        vector_q += empties((2, 2)) + [(quant_w1, whole(1, 0)), (quant_x, (2, 2)), (quant_x, (2, 0)), by("vector", whole(1, 1))]
-        vector_q += [(quant_w1, whole(1, 2)), (quant_w1, whole(1, 1)), (quant_w1, high(1, 3)), (quant_w1, low(1, 3))]
+        vector_q += empties((2, 2)) + [(quant_w1, whole(1, 0)), (quant_x, (2, 2)), by("vector", whole(1, 1)), (quant_x, (2, 0))]
+        vector_q += [(quant_w1, whole(1, 1)), (quant_w1, whole(1, 2)), (quant_w1, high(1, 3)), (quant_w1, low(1, 3))]
         vector_q += empties((3, 4)) + [(weave_h, FRONT, 0, "vector"), (quant_x, (3, 4)), (quant_h, FRONT, 0)]
         vector_q += [(weave_w2, W2_PIECES[2], "vector"), (quant_w2, W2_PIECES[1])] + empties((3, 2))
         vector_q += [(quant_w2, W2_PIECES[2]), (quant_w2, W2_PIECES[0]), (quant_x, (3, 2))]
@@ -415,8 +428,12 @@ def tile_rssm_pa_kernel(tc, prev_state, prev_action, obs_bytes, obs_scale, eps,
                 return [(load_w1,) + a[0][:2]]
             if f == quant_w1:
                 return [step for step in everything if step[0] == weave_w1 and step[1] == a[0]]
+            if f == first_pass:
+                return w1_steps(quant_w1, 0, ORDER[0]) + [(quant_first,) + a]
+            if f == quant_first:
+                return [emptier(a[0], ORDER[0])]
             if f == front_pass:
-                return w1_steps(quant_w1, *a) + [(quant_x, ("front", a[1]))]
+                return w1_steps(quant_w1, *a) + [(quant_x, ("front", a[1])) if a[1] != ORDER[0] or (quant_first, 1) not in everything else (quant_first, 1)]
             if f == fill_bank:
                 quarter = GROUPS[a[0][0]][0]
                 return [s for g in ORDER for s in w1_steps(quant_w1, a[1], g) + [(quant_x, pair_of(quarter, g)[0])]]
@@ -461,9 +478,11 @@ def tile_rssm_pa_kernel(tc, prev_state, prev_action, obs_bytes, obs_scale, eps,
                 return [(tag, DEPTH[tag], [(quant_w2 if f == weave_w2 else quant_h,) + a[:-1]])]
             if f in (drain, product):
                 pair = pair_of(*a)[0]
-                return [] if ("x", pair) in woven else [("woven_x", DEPTH["woven_x"], [(quant_x, pair)])]
+                return [] if ("x", pair) in woven else [("woven_x", DEPTH["woven_x"], [(quant_x, pair) if pair != ("front", ORDER[0]) or (quant_first, 1) not in everything else (quant_first, 1)])]
             if f == turn:
                 return [(turn_tag(*a), 4, [emptier(*a)])]
+            if f == first_pass and a[0] == 0:
+                return [("acc", 4, [(relu, FRONT, 0, t - t % 2)]) for t in range(4)]
             if f == front_pass and a[1] == ORDER[0]:
                 return [("acc", 4, [(relu, FRONT, a[0], t - t % 2)]) for t in range(4)]
             if f == fill_bank:

@@ -32,8 +32,8 @@ SPLIT = 2 * L - KP
 ALL_PASSES, FIRST_PASS, SECOND_PASS = (0, 1), (0,), (1,)
 W2_PIECES = tuple((g, c0, min(KP, 2 * L - c0)) for g in range(G2) for c0 in (0, KP))
 RUNS = KP // 8
-ORDER = (4, 5, 0, 2, 1, 3)
-DEPTH = {"wraw": 7, "woven_w": 3, "woven_g": 1, "woven_v": 1, "woven_s": 2, "woven_x": 3, "res": 4,
+ORDER = ((4, 5, 0, 2, 1, 3), (4, 5, 0, 2, 3, 1))
+DEPTH = {"wraw": 6, "woven_w": 3, "woven_g": 1, "woven_v": 2, "woven_s": 2, "woven_x": 3, "res": 4,
          "state1": 4, "state2": 1, "wide2": 8, "wide4": 4, "obs2": 2, "obs4": 2}
 HIDDEN_DEPTH = {2 * QT: 2, QT: 3, P: 2}
 HEAD_RUNS = 44
@@ -174,7 +174,7 @@ def tile_rssm_pa_kernel(tc, prev_state, prev_action, obs_bytes, obs_scale, eps,
                                   scales=xs[grp][:, g0:g0 + n, :].rearrange("p g n -> p (g n)"), in_=woven["x", pair][:])
 
         def quant_first(q):
-            g, cols = ORDER[0], slice(QT * q, QT * q + QT)
+            g, cols = ORDER[0][0], slice(QT * q, QT * q + QT)
             nc.vector.quantize_mx(out=xc[0][:, g, cols].bitcast(FP8X4), scales=xs[0][:, g, cols], in_=x_half(q, g))
 
         def weave_w1(part, engine, r0, r1):
@@ -219,11 +219,11 @@ def tile_rssm_pa_kernel(tc, prev_state, prev_action, obs_bytes, obs_scale, eps,
             cols = slice(KP * half + P * t, KP * half + P * t + P)
             nc.tensor.matmul_mx(out=sums, lhsT=w1c[:, g, cols].bitcast(FP8X4), lhsT_scale=w1s[:, g, cols],
                                 rhs=xc[grp][:, g, r0:r0 + n].bitcast(FP8X4), rhs_scale=xs[grp][:, g, r0:r0 + n],
-                                start=(g == ORDER[0] and r0 % KP == 0 or g == ORDER[0] and grp > 0), stop=(g == ORDER[-1]))
+                                start=(g == ORDER[half][0] and (grp > 0 or r0 == 0)), stop=(g == ORDER[half][-1]))
 
         def front_pass(half, g):
             for t in range(4):
-                if g == ORDER[0]:
+                if g == ORDER[half][0]:
                     acc = psum.tile([P, KP], F32, name="acc")
                     banks[FRONT, half, t] = acc[:]
                 mm1(FRONT, half, t, g)
@@ -233,7 +233,7 @@ def tile_rssm_pa_kernel(tc, prev_state, prev_action, obs_bytes, obs_scale, eps,
                 if q == 0:
                     acc = psum.tile([P, KP], F32, name="acc")
                     banks[FRONT, 0, t] = acc[:]
-                mm1((0, QT * q, QT), 0, t, ORDER[0])
+                mm1((0, QT * q, QT), 0, t, ORDER[0][0])
 
         def bank_start(span, t):
             return t - t % (KP // span[2])
@@ -243,7 +243,7 @@ def tile_rssm_pa_kernel(tc, prev_state, prev_action, obs_bytes, obs_scale, eps,
             acc = psum.tile([P, KP // n, n], F32, name=bank_tag(span, half))
             for t in range(t0, t0 + KP // n):
                 banks[span, half, t] = acc[:, t - t0, :]
-                for g in ORDER:
+                for g in ORDER[half]:
                     mm1(span, half, t, g)
 
         def relu(span, half, t0):
@@ -353,13 +353,13 @@ def tile_rssm_pa_kernel(tc, prev_state, prev_action, obs_bytes, obs_scale, eps,
             sync_q += [(load_obs, q, 2), (load_action, 2 * q), (load_action, 2 * q + 1)]
         sync_q += [(load_w1, 0, 0), (load_w1, 0, 2), (load_state, 0, 1), (load_state, 1, 1), (load_w1, 0, 1), (load_w1, 0, 3), (load_b1,)]
         sync_q += rows_of(2) + [(load_w1, 1, g) for g in (4, 5, 0)] + [(load_obs, 3, 4)] + [(load_w1, 1, g) for g in (3, 1, 2)] + rows_of(3)[1:]
-        sync_q += [(load_w2, piece) for piece in W2_PIECES] + [(load_b2,), (load_eps,)] + stores
+        sync_q += [(load_w2, piece) for piece in W2_PIECES[1::-1] + W2_PIECES[2:]] + [(load_b2,), (load_eps,)] + stores
 
         tensor_q = [(turn, q, g) for q in GROUPS[0] for g in (4, 5)] + turns(front(0)) + turns(front(2)) + [(front_pass, 0, 4)]
         tensor_q += turns(front(1)) + [(front_pass, 0, 5)] + turns(front(3)) + [(front_pass, 0, 0), (front_pass, 0, 2)]
         tensor_q += turns((2, 4)) + [(front_pass, 0, 1)]
         tensor_q += [(front_pass, 0, 3)] + turns((2, 2)) + [(front_pass, 1, 4)] + turns((2, 0)) + [(front_pass, 1, 5)] + turns((3, 4)) + [(front_pass, 1, 0), (fill_bank, THIRD, 0, 0)]
-        tensor_q += [(front_pass, 1, 2), (front_pass, 1, 1), (front_pass, 1, 3), (fill_bank, THIRD, 0, 2)] + turns((3, 2))
+        tensor_q += [(front_pass, 1, 2), (front_pass, 1, 3), (front_pass, 1, 1), (fill_bank, THIRD, 0, 2)] + turns((3, 2))
         tensor_q += [(fill_bank, THIRD, 1, 0)] + turns((3, 0)) + [(fill_bank, THIRD, 1, 2), (heads, 0), (heads, 1)]
 
         gpsimd_q = [by("gpsimd", low(0, g)) for g in (5, 2, 3)] + [by("gpsimd", low(1, g)) for g in (4, 3)]
@@ -373,17 +373,16 @@ def tile_rssm_pa_kernel(tc, prev_state, prev_action, obs_bytes, obs_scale, eps,
         scalar_q += [(weave_w2, W2_PIECES[0], "scalar")] + relus(FRONT, 1) + [(relu, THIRD, 0, 2)]
         scalar_q += [(weave_h, FRONT, 1, "scalar")] + empties((3, 0)) + relus(THIRD, 1)
 
-        vector_q = [by("vector", first, 0, HEAD_RUNS), (product, 0, 4), (product, 0, 5), (quant_w1, first), (product, 1, 4), (product, 1, 5)]
-        vector_q += [(quant_w1, high(0, 5)), (quant_x, front(4)), (quant_x, front(5)), (quant_x, front(0)), (quant_w1, low(0, 5))]
-        vector_q += empties(front(2)) + [(quant_w1, whole(0, 0)), (quant_x, front(2)), (quant_w1, high(0, 2)), (quant_x, front(1)), (quant_w1, low(0, 2))]
-        vector_q += empties(front(3)) + [(quant_w1, whole(0, 1)), (quant_x, front(3)), (quant_w1, high(0, 3)), (quant_w1, low(0, 3))]
-        vector_q += empties((2, 4)) + [(quant_w1, high(1, 4)), (quant_w1, low(1, 4)), by("vector", second), (quant_x, (2, 4)), (quant_w1, second)]
-        vector_q += empties((2, 2)) + [(quant_w1, whole(1, 0)), (quant_x, (2, 2)), by("vector", whole(1, 1)), (quant_x, (2, 0))]
-        vector_q += [(quant_w1, whole(1, 1)), (quant_w1, whole(1, 2)), (quant_w1, high(1, 3)), (quant_w1, low(1, 3))]
-        vector_q += empties((3, 4)) + [(weave_h, FRONT, 0, "vector"), (quant_x, (3, 4)), (quant_h, FRONT, 0)]
-        vector_q += [(weave_w2, W2_PIECES[2], "vector"), (quant_w2, W2_PIECES[1])] + empties((3, 2))
-        vector_q += [(quant_w2, W2_PIECES[2]), (quant_w2, W2_PIECES[0]), (quant_x, (3, 2))]
-        vector_q += [(quant_w2, W2_PIECES[3]), (quant_h, FRONT, 1), (quant_x, (3, 0))]
+        vector_q = [by("vector", first, 0, HEAD_RUNS), (product, 0, 4), (quant_w1, first), (product, 0, 5), (product, 1, 4), (product, 1, 5)]
+        vector_q += [(quant_w1, high(0, 5)), (quant_x, front(4)), (quant_x, front(5)), (quant_w1, low(0, 5)), (quant_x, front(0))]
+        vector_q += empties(front(2)) + [(quant_w1, whole(0, 0)), (quant_x, front(2)), (quant_w1, high(0, 2)), (quant_w1, low(0, 2)), (quant_x, front(1))]
+        vector_q += empties(front(3)) + [(quant_w1, whole(0, 1)), (quant_x, front(3)), (quant_w1, low(0, 3)), (quant_w1, high(0, 3))]
+        vector_q += empties((2, 4)) + [(quant_w1, high(1, 4)), (quant_w1, low(1, 4)), by("vector", second), (quant_w1, second), (quant_x, (2, 4))]
+        vector_q += empties((2, 2)) + [(quant_w1, whole(1, 0)), (quant_x, (2, 2)), (quant_x, (2, 0)), by("vector", whole(1, 1))]
+        vector_q += [(quant_w1, whole(1, 2)), (quant_w1, high(1, 3)), (quant_w1, low(1, 3)), (quant_w1, whole(1, 1))]
+        vector_q += empties((3, 4)) + [(weave_h, FRONT, 0, "vector"), (quant_x, (3, 4)), (weave_w2, W2_PIECES[2], "vector")]
+        vector_q += [(quant_h, FRONT, 0), (quant_w2, W2_PIECES[0]), (quant_w2, W2_PIECES[1]), (quant_w2, W2_PIECES[2])] + empties((3, 2))
+        vector_q += [(quant_h, FRONT, 1), (quant_w2, W2_PIECES[3]), (quant_x, (3, 2)), (quant_x, (3, 0))]
 
         after_root = [[(weave_h, THIRD, 0, "scalar")], [(relu, LAST, 0, 0), (weave_h, THIRD, 1, "scalar")],
                       [(relu, LAST, 0, 2), (weave_h, LAST, 0, "scalar")],
@@ -429,17 +428,17 @@ def tile_rssm_pa_kernel(tc, prev_state, prev_action, obs_bytes, obs_scale, eps,
             if f == quant_w1:
                 return [step for step in everything if step[0] == weave_w1 and step[1] == a[0]]
             if f == first_pass:
-                return w1_steps(quant_w1, 0, ORDER[0]) + [(quant_first,) + a]
+                return w1_steps(quant_w1, 0, ORDER[0][0]) + [(quant_first,) + a]
             if f == quant_first:
-                return [emptier(a[0], ORDER[0])]
+                return [emptier(a[0], ORDER[0][0])]
             if f == front_pass:
-                return w1_steps(quant_w1, *a) + [(quant_x, ("front", a[1])) if a[1] != ORDER[0] or (quant_first, 1) not in everything else (quant_first, 1)]
+                return w1_steps(quant_w1, *a) + [(quant_x, ("front", a[1])) if a[1] != ORDER[0][0] or (quant_first, 1) not in everything else (quant_first, 1)]
             if f == fill_bank:
                 quarter = GROUPS[a[0][0]][0]
-                return [s for g in ORDER for s in w1_steps(quant_w1, a[1], g) + [(quant_x, pair_of(quarter, g)[0])]]
+                return [s for g in range(G1) for s in w1_steps(quant_w1, a[1], g) + [(quant_x, pair_of(quarter, g)[0])]]
             if f == relu:
                 span, half, t0 = a
-                sums = (front_pass, half, ORDER[-1]) if span == FRONT else (fill_bank, span, half, bank_start(span, t0))
+                sums = (front_pass, half, ORDER[half][-1]) if span == FRONT else (fill_bank, span, half, bank_start(span, t0))
                 return [(load_b1,), sums]
             if f == heads:
                 passes = a[1] if len(a) > 1 else ALL_PASSES
@@ -478,12 +477,12 @@ def tile_rssm_pa_kernel(tc, prev_state, prev_action, obs_bytes, obs_scale, eps,
                 return [(tag, DEPTH[tag], [(quant_w2 if f == weave_w2 else quant_h,) + a[:-1]])]
             if f in (drain, product):
                 pair = pair_of(*a)[0]
-                return [] if ("x", pair) in woven else [("woven_x", DEPTH["woven_x"], [(quant_x, pair) if pair != ("front", ORDER[0]) or (quant_first, 1) not in everything else (quant_first, 1)])]
+                return [] if ("x", pair) in woven else [("woven_x", DEPTH["woven_x"], [(quant_x, pair) if pair != ("front", ORDER[0][0]) or (quant_first, 1) not in everything else (quant_first, 1)])]
             if f == turn:
                 return [(turn_tag(*a), 4, [emptier(*a)])]
             if f == first_pass and a[0] == 0:
                 return [("acc", 4, [(relu, FRONT, 0, t - t % 2)]) for t in range(4)]
-            if f == front_pass and a[1] == ORDER[0]:
+            if f == front_pass and a[1] == ORDER[a[0]][0]:
                 return [("acc", 4, [(relu, FRONT, a[0], t - t % 2)]) for t in range(4)]
             if f == fill_bank:
                 return [(bank_tag(a[0], a[1]), 4, [(relu, a[0], a[1], a[2] + KP // a[0][2] - 2)])]

@@ -37,6 +37,8 @@ DEPTH = {"wraw": 6, "woven_w": 3, "woven_g": 1, "woven_v": 2, "woven_s": 2, "wov
          "state1": 4, "state2": 1, "wide2": 8, "wide4": 4, "obs2": 2, "obs4": 2}
 HIDDEN_DEPTH = {2 * QT: 2, QT: 3, P: 2}
 HEAD_RUNS = 44
+FRONT_A, FRONT_B = (0, 0, QT), (0, QT, QT)
+POOL_RUNS = 52
 
 
 def tile_rssm_pa_kernel(tc, prev_state, prev_action, obs_bytes, obs_scale, eps,
@@ -221,8 +223,8 @@ def tile_rssm_pa_kernel(tc, prev_state, prev_action, obs_bytes, obs_scale, eps,
                                 rhs=xc[grp][:, g, r0:r0 + n].bitcast(FP8X4), rhs_scale=xs[grp][:, g, r0:r0 + n],
                                 start=(g == ORDER[half][0] and (grp > 0 or r0 == 0)), stop=(g == ORDER[half][-1]))
 
-        def front_pass(half, g):
-            for t in range(4):
+        def front_pass(half, g, t0=0, t1=4):
+            for t in range(t0, t1):
                 if g == ORDER[half][0]:
                     acc = psum.tile([P, KP], F32, name="acc")
                     banks[FRONT, half, t] = acc[:]
@@ -255,7 +257,9 @@ def tile_rssm_pa_kernel(tc, prev_state, prev_action, obs_bytes, obs_scale, eps,
                                      bias=b1_cols[:, half, t:t + 1])
 
         def weave_h(span, half, engine):
-            weave((span, half), hidden[span, half][:], engine)
+            grp, r0, n = span
+            src = hidden[FRONT, half][:, :, r0:r0 + n] if grp == 0 else hidden[span, half][:]
+            weave((span, half), src, engine)
 
         def quant_h(span, half):
             grp, r0, n = span
@@ -263,7 +267,8 @@ def tile_rssm_pa_kernel(tc, prev_state, prev_action, obs_bytes, obs_scale, eps,
                                   in_=woven[span, half])
 
         def spans_of(n):
-            front, third = [(FRONT, 0), (FRONT, 1)], [(THIRD, 0), (THIRD, 1)]
+            piece = FRONT if (FRONT, 0) in weaver else (0, QT * (n // 2), QT)
+            front, third = [(piece, 0), (piece, 1)], [(THIRD, 0), (THIRD, 1)]
             return front if n < 4 else third if n < 6 else [(LAST, 0), ((LAST_A, LAST_B)[n - 6], 1)]
 
         def heads(n, passes=ALL_PASSES):
@@ -327,10 +332,10 @@ def tile_rssm_pa_kernel(tc, prev_state, prev_action, obs_bytes, obs_scale, eps,
             return (half, g, 0, 4, "woven_w")
 
         def low(half, g):
-            return (half, g, 0, 2, "woven_g")
+            return (half, g, 0, 3, "woven_g")
 
         def high(half, g):
-            return (half, g, 2, 4, "woven_w")
+            return (half, g, 3, 4, "woven_w")
 
         def by(engine, part, r0=0, r1=RUNS):
             return (weave_w1, part, engine, r0, r1)
@@ -347,58 +352,59 @@ def tile_rssm_pa_kernel(tc, prev_state, prev_action, obs_bytes, obs_scale, eps,
             stores += [(store_std, n), (store_mean, n)] + ([(store_sample, n - 1)] if n else [])
         stores += [(store_sample,) + part for part in halves]
 
+        early, late = (0, 5, 0, 2, "woven_g"), (0, 5, 2, 4, "woven_w")
         first, second = (0, 4, 0, 4, "woven_g"), (1, 5, 0, 4, "woven_g")
         sync_q = [(load_obs, 0, 4), (load_w1, 0, 4), (load_scales,), (load_obs, 1, 4), (load_w1, 0, 5), (load_state, 0, 0), (load_state, 1, 0)]
         for q in GROUPS[0]:
             sync_q += [(load_obs, q, 2), (load_action, 2 * q), (load_action, 2 * q + 1)]
-        sync_q += [(load_w1, 0, 0), (load_w1, 0, 2), (load_state, 0, 1), (load_state, 1, 1), (load_w1, 0, 1), (load_w1, 0, 3), (load_b1,)]
-        sync_q += rows_of(2) + [(load_w1, 1, g) for g in (4, 5, 0)] + [(load_obs, 3, 4)] + [(load_w1, 1, g) for g in (3, 1, 2)] + rows_of(3)[1:]
+        sync_q += [(load_w1, 0, 0), (load_w1, 0, 2), (load_state, 0, 1), (load_state, 1, 1), (load_obs, 2, 4), (load_w1, 0, 1), (load_w1, 0, 3), (load_b1,)]
+        sync_q += rows_of(2)[1:] + [(load_w1, 1, g) for g in (4, 5, 0)] + [(load_obs, 3, 4)] + [(load_w1, 1, g) for g in (3, 1, 2)] + rows_of(3)[1:]
         sync_q += [(load_w2, piece) for piece in W2_PIECES[1::-1] + W2_PIECES[2:]] + [(load_b2,), (load_eps,)] + stores
 
-        tensor_q = [(turn, q, g) for q in GROUPS[0] for g in (4, 5)] + turns(front(0)) + turns(front(2)) + [(front_pass, 0, 4)]
-        tensor_q += turns(front(1)) + [(front_pass, 0, 5)] + turns(front(3)) + [(front_pass, 0, 0), (front_pass, 0, 2)]
-        tensor_q += turns((2, 4)) + [(front_pass, 0, 1)]
-        tensor_q += [(front_pass, 0, 3)] + turns((2, 2)) + [(front_pass, 1, 4)] + turns((2, 0)) + [(front_pass, 1, 5)] + turns((3, 4)) + [(front_pass, 1, 0), (fill_bank, THIRD, 0, 0)]
+        tensor_q = [(turn, q, g) for q in GROUPS[0] for g in (4, 5)] + turns(front(0)) + [(front_pass, 0, 4)] + turns(front(2))
+        tensor_q += [(front_pass, 0, 5, 0, 2)] + turns(front(1)) + [(front_pass, 0, 5, 2, 4), (turn, 0, 3), (front_pass, 0, 0), (turn, 1, 3), (turn, 2, 4), (front_pass, 0, 2)]
+        tensor_q += [(turn, 2, 5), (front_pass, 0, 1)]
+        tensor_q += [(front_pass, 0, 3, 0, 2)] + turns((2, 2)) + [(front_pass, 0, 3, 2, 4)] + [(front_pass, 1, 4)] + turns((2, 0)) + [(front_pass, 1, 5, 0, 2), (turn, 3, 4), (front_pass, 1, 5, 2, 4), (turn, 3, 5)] + [(front_pass, 1, 0), (fill_bank, THIRD, 0, 0)]
         tensor_q += [(front_pass, 1, 2), (front_pass, 1, 3), (front_pass, 1, 1), (fill_bank, THIRD, 0, 2)] + turns((3, 2))
         tensor_q += [(fill_bank, THIRD, 1, 0)] + turns((3, 0)) + [(fill_bank, THIRD, 1, 2), (heads, 0), (heads, 1)]
 
-        gpsimd_q = [by("gpsimd", low(0, g)) for g in (5, 2, 3)] + [by("gpsimd", low(1, g)) for g in (4, 3)]
-        gpsimd_q += [(weave_w2, W2_PIECES[1], "gpsimd"), (weave_w2, W2_PIECES[3], "gpsimd")]
+        gpsimd_q = [by("gpsimd", early)] + [by("gpsimd", low(0, g), 0, POOL_RUNS) for g in (2, 3)] + [by("gpsimd", low(1, g), 0, POOL_RUNS) for g in (4, 3)]
+        gpsimd_q += [(weave_w2, W2_PIECES[1], "gpsimd"), (weave_h, FRONT_B, 0, "gpsimd")]
 
-        scalar_q = widens(0, 4) + [by("scalar", first, HEAD_RUNS)] + widens(1, 4) + [by("scalar", high(0, 5))] + widens(0, 2) + [(drain, 0, 0)] + widens(1, 2) + [(drain, 1, 0)]
-        scalar_q += [by("scalar", whole(0, 0)), by("scalar", high(0, 2))] + empties(front(1)) + [by("scalar", whole(0, 1))]
-        scalar_q += widens(2, 4) + [by("scalar", high(0, 3)), by("scalar", high(1, 4))] + widens(2, 2)
-        scalar_q += relus(FRONT, 0) + widens(3, 4) + [by("scalar", whole(1, 0))] + empties((2, 0))
+        scalar_q = widens(0, 4) + [by("scalar", first, HEAD_RUNS)] + widens(1, 4) + [by("scalar", late)] + widens(0, 2) + [(drain, 0, 0)] + widens(1, 2) + [(drain, 1, 0)]
+        scalar_q += [by("scalar", whole(0, 0)), by("scalar", high(0, 2))] + empties(front(1)) + widens(2, 4)
+        scalar_q += [by("scalar", whole(0, 1)), by("scalar", high(0, 3)), by("scalar", high(1, 4))] + widens(2, 2)
+        scalar_q += [(relu, FRONT, 0, 0), (widen, 6, 4, "scalar"), (relu, FRONT, 0, 2), (widen, 7, 4, "scalar")] + [by("scalar", whole(1, 0))] + empties((2, 0))
         scalar_q += [by("scalar", whole(1, 2)), by("scalar", high(1, 3))] + widens(3, 2) + [(relu, THIRD, 0, 0)]
-        scalar_q += [(weave_w2, W2_PIECES[0], "scalar")] + relus(FRONT, 1) + [(relu, THIRD, 0, 2)]
-        scalar_q += [(weave_h, FRONT, 1, "scalar")] + empties((3, 0)) + relus(THIRD, 1)
+        scalar_q += [(weave_w2, W2_PIECES[0], "scalar"), (weave_w2, W2_PIECES[3], "scalar")] + relus(FRONT, 1) + [(relu, THIRD, 0, 2)]
+        scalar_q += [(weave_h, FRONT_A, 1, "scalar")] + empties((3, 0)) + [(weave_h, FRONT_B, 1, "scalar")] + relus(THIRD, 1)
 
-        vector_q = [by("vector", first, 0, HEAD_RUNS), (product, 0, 4), (quant_w1, first), (product, 0, 5), (product, 1, 4), (product, 1, 5)]
-        vector_q += [(quant_w1, high(0, 5)), (quant_x, front(4)), (quant_x, front(5)), (quant_w1, low(0, 5)), (quant_x, front(0))]
-        vector_q += empties(front(2)) + [(quant_w1, whole(0, 0)), (quant_x, front(2)), (quant_w1, high(0, 2)), (quant_w1, low(0, 2)), (quant_x, front(1))]
-        vector_q += empties(front(3)) + [(quant_w1, whole(0, 1)), (quant_x, front(3)), (quant_w1, low(0, 3)), (quant_w1, high(0, 3))]
-        vector_q += empties((2, 4)) + [(quant_w1, high(1, 4)), (quant_w1, low(1, 4)), by("vector", second), (quant_w1, second), (quant_x, (2, 4))]
-        vector_q += empties((2, 2)) + [(quant_w1, whole(1, 0)), (quant_x, (2, 2)), (quant_x, (2, 0)), by("vector", whole(1, 1))]
+        vector_q = [by("vector", first, 0, HEAD_RUNS), (product, 0, 4), (quant_w1, first), (product, 0, 5), (product, 1, 4), (quant_x, front(4)), (product, 1, 5)]
+        vector_q += [(quant_w1, late), (quant_x, front(5)), (quant_w1, early), (quant_x, front(0))]
+        vector_q += empties(front(2)) + [by("vector", low(0, 2), POOL_RUNS), (quant_w1, whole(0, 0)), (quant_x, front(2)), (quant_w1, high(0, 2)), (quant_w1, low(0, 2)), (quant_x, front(1))]
+        vector_q += empties(front(3)) + [by("vector", low(0, 3), POOL_RUNS), (quant_w1, whole(0, 1)), (quant_w1, high(0, 3)), (quant_w1, low(0, 3)), (quant_x, front(3))]
+        vector_q += empties((2, 4)) + [by("vector", low(1, 4), POOL_RUNS), (quant_w1, high(1, 4)), (quant_w1, low(1, 4)), by("vector", second), (quant_w1, second), (quant_x, (2, 4))]
+        vector_q += empties((2, 2)) + [by("vector", low(1, 3), POOL_RUNS), (quant_w1, whole(1, 0)), (quant_x, (2, 2)), (quant_x, (2, 0)), by("vector", whole(1, 1))]
         vector_q += [(quant_w1, whole(1, 2)), (quant_w1, high(1, 3)), (quant_w1, low(1, 3)), (quant_w1, whole(1, 1))]
-        vector_q += empties((3, 4)) + [(weave_h, FRONT, 0, "vector"), (quant_x, (3, 4)), (weave_w2, W2_PIECES[2], "vector")]
-        vector_q += [(quant_h, FRONT, 0), (quant_w2, W2_PIECES[0]), (quant_w2, W2_PIECES[1]), (quant_w2, W2_PIECES[2])] + empties((3, 2))
-        vector_q += [(quant_h, FRONT, 1), (quant_w2, W2_PIECES[3]), (quant_x, (3, 2)), (quant_x, (3, 0))]
+        vector_q += empties((3, 4)) + [(weave_h, FRONT_A, 0, "vector"), (quant_x, (3, 4)), (weave_w2, W2_PIECES[2], "vector")]
+        vector_q += [(quant_h, FRONT_A, 0), (quant_w2, W2_PIECES[0]), (quant_w2, W2_PIECES[3]), (quant_w2, W2_PIECES[1]), (quant_w2, W2_PIECES[2])] + empties((3, 2))
+        vector_q += [(quant_h, FRONT_A, 1), (quant_x, (3, 2)), (quant_x, (3, 0)), (quant_h, FRONT_B, 0)]
 
         after_root = [[(weave_h, THIRD, 0, "scalar")], [(relu, LAST, 0, 0), (weave_h, THIRD, 1, "scalar")],
-                      [(relu, LAST, 0, 2), (weave_h, LAST, 0, "scalar")],
-                      relus(LAST_A, 1) + [(weave_h, LAST_A, 1, "scalar")], [], [], [], []]
+                      [(relu, LAST, 0, 2)], [(weave_h, LAST, 0, "scalar")],
+                      relus(LAST_A, 1) + [(weave_h, LAST_A, 1, "scalar")], relus(LAST_B, 1), [], []]
         for n in range(NT):
-            scalar_q += (relus(LAST_B, 1) if n == 5 else []) + [(root, n)] + after_root[n]
-        after_tile = [[], [(quant_h, THIRD, 0)], [(quant_h, THIRD, 1)], [(quant_h, LAST, 0)], [(quant_h, LAST_A, 1)]]
+            scalar_q += [(root, n)] + after_root[n]
+        after_tile = [[(quant_h, FRONT_B, 1)], [(quant_h, THIRD, 0)], [(quant_h, THIRD, 1)], [], [(quant_h, LAST, 0)]]
         for n in range(NT - 3):
             vector_q += [(bias_wide, n)] + ([(noise, n - 1)] if n else []) + [(bias_narrow, n)]
             vector_q += ([(shift, n - 1)] if n else []) + after_tile[n]
-        vector_q += [(bias_wide, 5), (noise, 4), (bias_narrow, 5), (shift, 4), (weave_h, LAST_B, 1, "vector"), (bias_wide, 6), (quant_h, LAST_B, 1)]
-        vector_q += [(noise, 5), (bias_narrow, 6), (shift, 5), (bias_wide, 7), (noise, 6), (bias_narrow, 7), (shift, 6)]
+        vector_q += [(bias_wide, 5), (noise, 4), (bias_narrow, 5), (shift, 4), (quant_h, LAST_A, 1), (noise, 5), (weave_h, LAST_B, 1, "vector"), (bias_wide, 6), (quant_h, LAST_B, 1)]
+        vector_q += [(shift, 5), (bias_narrow, 6), (bias_wide, 7), (noise, 6), (bias_narrow, 7), (shift, 6)]
         vector_q += [(f,) + part for f in (noise, shift) for part in halves]
-        tensor_q += [(fill_bank, LAST, 0, 0), (heads, 2), (fill_bank, LAST, 0, 2), (heads, 3), (fill_bank, LAST_A, 1, 0), (heads, 4), (heads, 5)]
+        tensor_q += [(fill_bank, LAST, 0, 0), (heads, 2), (fill_bank, LAST, 0, 2), (heads, 3), (heads, 4), (fill_bank, LAST_A, 1, 0), (heads, 5)]
         tensor_q += [(fill_bank, LAST_B, 1, 0), (heads, NT - 2), (heads, NT - 1, FIRST_PASS), (heads, NT - 1, SECOND_PASS)]
-        behind = {by("gpsimd", low(1, 3)): [(quant_w1, second)]}
+        behind = {by("gpsimd", low(1, 3), 0, POOL_RUNS): [(quant_w1, second)]}
 
         everything = sync_q + tensor_q + scalar_q + vector_q + gpsimd_q
         weaver = {step[1:-1]: step for step in everything if step[0] in (weave_w2, weave_h)}
@@ -432,14 +438,16 @@ def tile_rssm_pa_kernel(tc, prev_state, prev_action, obs_bytes, obs_scale, eps,
             if f == quant_first:
                 return [emptier(a[0], ORDER[0][0])]
             if f == front_pass:
-                return w1_steps(quant_w1, *a) + [(quant_x, ("front", a[1])) if a[1] != ORDER[0][0] or (quant_first, 1) not in everything else (quant_first, 1)]
+                return w1_steps(quant_w1, *a[:2]) + [(quant_x, ("front", a[1])) if a[1] != ORDER[0][0] or (quant_first, 1) not in everything else (quant_first, 1)]
             if f == fill_bank:
                 quarter = GROUPS[a[0][0]][0]
                 return [s for g in range(G1) for s in w1_steps(quant_w1, a[1], g) + [(quant_x, pair_of(quarter, g)[0])]]
             if f == relu:
                 span, half, t0 = a
-                sums = (front_pass, half, ORDER[half][-1]) if span == FRONT else (fill_bank, span, half, bank_start(span, t0))
-                return [(load_b1,), sums]
+                if span != FRONT:
+                    return [(load_b1,), (fill_bank, span, half, bank_start(span, t0))]
+                last = [s for s in everything if s[:3] == (front_pass, half, ORDER[half][-1])]
+                return [(load_b1,)] + [s for s in last if len(s) == 3 or s[3] == t0]
             if f == heads:
                 passes = a[1] if len(a) > 1 else ALL_PASSES
                 pieces = [(quant_h, span, half) for span, half in spans_of(a[0]) if half in passes]
@@ -447,7 +455,7 @@ def tile_rssm_pa_kernel(tc, prev_state, prev_action, obs_bytes, obs_scale, eps,
             if f == bias_wide:
                 return [(heads, a[0], SECOND_PASS) if a[0] == NT - 1 else (heads, a[0]), (load_b2,)]
             if f == weave_h:
-                return relus(a[0], a[1])
+                return relus(FRONT if a[0][0] == 0 else a[0], a[1])
             if f in (quant_w2, quant_h):
                 return [weaver[a]]
             simple = {drain: [(turn,) + a], weave_w2: [(load_w2,) + a[:1]], bias_narrow: [(bias_wide,) + a],
@@ -487,7 +495,7 @@ def tile_rssm_pa_kernel(tc, prev_state, prev_action, obs_bytes, obs_scale, eps,
             if f == fill_bank:
                 return [(bank_tag(a[0], a[1]), 4, [(relu, a[0], a[1], a[2] + KP // a[0][2] - 2)])]
             if f == relu and a[2] == 0:
-                return [(("hidden", a[0][2]), HIDDEN_DEPTH[a[0][2]], [weaver[a[:2]]])]
+                return [(("hidden", a[0][2]), HIDDEN_DEPTH[a[0][2]], [s for k, s in weaver.items() if k == a[:2] or (a[0] == FRONT and k[0][0] == 0 and len(k) == 2 and k[1] == a[1])])]
             if f == heads and a[1:] != (SECOND_PASS,):
                 return [("tp", 4, [(bias_wide, a[0])]), ("tp", 4, [(bias_narrow, a[0])])]
             if f == bias_wide:

@@ -38,7 +38,7 @@ DEPTH = {"wraw": 6, "woven_w": 3, "woven_g": 1, "woven_v": 2, "woven_s": 2, "wov
 HIDDEN_DEPTH = {2 * QT: 2, QT: 3, P: 2}
 HEAD_RUNS = 44
 FRONT_A, FRONT_B = (0, 0, QT), (0, QT, QT)
-POOL_RUNS = 52
+POOL_RUNS = 40
 
 
 def tile_rssm_pa_kernel(tc, prev_state, prev_action, obs_bytes, obs_scale, eps,
@@ -361,29 +361,29 @@ def tile_rssm_pa_kernel(tc, prev_state, prev_action, obs_bytes, obs_scale, eps,
         sync_q += rows_of(2)[1:] + [(load_w1, 1, g) for g in (4, 5, 0)] + [(load_obs, 3, 4)] + [(load_w1, 1, g) for g in (3, 1, 2)] + rows_of(3)[1:]
         sync_q += [(load_w2, piece) for piece in W2_PIECES[1::-1] + W2_PIECES[2:]] + [(load_b2,), (load_eps,)] + stores
 
-        tensor_q = [(turn, q, g) for q in GROUPS[0] for g in (4, 5)] + turns(front(0)) + [(front_pass, 0, 4)] + turns(front(2))
+        tensor_q = [(turn, q, g) for q in GROUPS[0] for g in (4, 5)] + turns(front(0)) + [(turn, 0, 2), (front_pass, 0, 4, 0, 2), (turn, 1, 2), (front_pass, 0, 4, 2, 4)]
         tensor_q += [(front_pass, 0, 5, 0, 2)] + turns(front(1)) + [(front_pass, 0, 5, 2, 4), (turn, 0, 3), (front_pass, 0, 0), (turn, 1, 3), (turn, 2, 4), (front_pass, 0, 2)]
         tensor_q += [(turn, 2, 5), (front_pass, 0, 1)]
         tensor_q += [(front_pass, 0, 3, 0, 2)] + turns((2, 2)) + [(front_pass, 0, 3, 2, 4)] + [(front_pass, 1, 4)] + turns((2, 0)) + [(front_pass, 1, 5, 0, 2), (turn, 3, 4), (front_pass, 1, 5, 2, 4), (turn, 3, 5)] + [(front_pass, 1, 0), (fill_bank, THIRD, 0, 0)]
         tensor_q += [(front_pass, 1, 2), (front_pass, 1, 3), (front_pass, 1, 1), (fill_bank, THIRD, 0, 2)] + turns((3, 2))
         tensor_q += [(fill_bank, THIRD, 1, 0)] + turns((3, 0)) + [(fill_bank, THIRD, 1, 2), (heads, 0), (heads, 1)]
 
-        gpsimd_q = [by("gpsimd", early)] + [by("gpsimd", low(0, g), 0, POOL_RUNS) for g in (2, 3)] + [by("gpsimd", low(1, g), 0, POOL_RUNS) for g in (4, 3)]
+        gpsimd_q = [by("gpsimd", early)] + [by("gpsimd", low(0, g), 0, POOL_RUNS) for g in (2, 3)] + [by("gpsimd", (1, 4, 0, 2, "woven_g")), by("gpsimd", low(1, 3), 0, POOL_RUNS)]
         gpsimd_q += [(weave_w2, W2_PIECES[1], "gpsimd"), (weave_h, FRONT_B, 0, "gpsimd")]
 
         scalar_q = widens(0, 4) + [by("scalar", first, HEAD_RUNS)] + widens(1, 4) + [by("scalar", late)] + widens(0, 2) + [(drain, 0, 0)] + widens(1, 2) + [(drain, 1, 0)]
         scalar_q += [by("scalar", whole(0, 0)), by("scalar", high(0, 2))] + empties(front(1)) + widens(2, 4)
-        scalar_q += [by("scalar", whole(0, 1)), by("scalar", high(0, 3)), by("scalar", high(1, 4))] + widens(2, 2)
+        scalar_q += [by("scalar", whole(0, 1)), by("scalar", high(0, 3)), by("scalar", (1, 4, 2, 4, "woven_w"))] + widens(2, 2)
         scalar_q += [(relu, FRONT, 0, 0), (widen, 6, 4, "scalar"), (relu, FRONT, 0, 2), (widen, 7, 4, "scalar")] + [by("scalar", whole(1, 0))] + empties((2, 0))
         scalar_q += [by("scalar", whole(1, 2)), by("scalar", high(1, 3))] + widens(3, 2) + [(relu, THIRD, 0, 0)]
         scalar_q += [(weave_w2, W2_PIECES[0], "scalar"), (weave_w2, W2_PIECES[3], "scalar")] + relus(FRONT, 1) + [(relu, THIRD, 0, 2)]
         scalar_q += [(weave_h, FRONT_A, 1, "scalar")] + empties((3, 0)) + [(weave_h, FRONT_B, 1, "scalar")] + relus(THIRD, 1)
 
-        vector_q = [by("vector", first, 0, HEAD_RUNS), (product, 0, 4), (quant_w1, first), (product, 0, 5), (product, 1, 4), (quant_x, front(4)), (product, 1, 5)]
-        vector_q += [(quant_w1, late), (quant_x, front(5)), (quant_w1, early), (quant_x, front(0))]
-        vector_q += empties(front(2)) + [by("vector", low(0, 2), POOL_RUNS), (quant_w1, whole(0, 0)), (quant_x, front(2)), (quant_w1, high(0, 2)), (quant_w1, low(0, 2)), (quant_x, front(1))]
-        vector_q += empties(front(3)) + [by("vector", low(0, 3), POOL_RUNS), (quant_w1, whole(0, 1)), (quant_w1, high(0, 3)), (quant_w1, low(0, 3)), (quant_x, front(3))]
-        vector_q += empties((2, 4)) + [by("vector", low(1, 4), POOL_RUNS), (quant_w1, high(1, 4)), (quant_w1, low(1, 4)), by("vector", second), (quant_w1, second), (quant_x, (2, 4))]
+        vector_q = [by("vector", first, 0, HEAD_RUNS), (product, 0, 4), (quant_w1, first), (product, 0, 5), (product, 1, 4), (product, 1, 5)]
+        vector_q += [(quant_x, front(4)), (quant_w1, late), (quant_w1, early), (quant_x, front(5))]
+        vector_q += empties(front(2)) + [(quant_x, front(0)), (quant_w1, whole(0, 0)), by("vector", low(0, 2), POOL_RUNS), (quant_w1, high(0, 2)), (quant_w1, low(0, 2)), (quant_x, front(2))]
+        vector_q += empties(front(3)) + [(quant_x, front(1)), (quant_w1, whole(0, 1)), by("vector", low(0, 3), POOL_RUNS), (quant_w1, high(0, 3)), (quant_w1, low(0, 3)), (quant_x, front(3))]
+        vector_q += empties((2, 4)) + [(quant_w1, (1, 4, 2, 4, "woven_w")), (quant_w1, (1, 4, 0, 2, "woven_g")), by("vector", second), (quant_x, (2, 4)), (quant_w1, second)]
         vector_q += empties((2, 2)) + [by("vector", low(1, 3), POOL_RUNS), (quant_w1, whole(1, 0)), (quant_x, (2, 2)), (quant_x, (2, 0)), by("vector", whole(1, 1))]
         vector_q += [(quant_w1, whole(1, 2)), (quant_w1, high(1, 3)), (quant_w1, low(1, 3)), (quant_w1, whole(1, 1))]
         vector_q += empties((3, 4)) + [(weave_h, FRONT_A, 0, "vector"), (quant_x, (3, 4)), (weave_w2, W2_PIECES[2], "vector")]
@@ -491,7 +491,7 @@ def tile_rssm_pa_kernel(tc, prev_state, prev_action, obs_bytes, obs_scale, eps,
             if f == first_pass and a[0] == 0:
                 return [("acc", 4, [(relu, FRONT, 0, t - t % 2)]) for t in range(4)]
             if f == front_pass and a[1] == ORDER[a[0]][0]:
-                return [("acc", 4, [(relu, FRONT, a[0], t - t % 2)]) for t in range(4)]
+                return [("acc", 4, [(relu, FRONT, a[0], t - t % 2)]) for t in range(*(a[2:] or (4,)))]
             if f == fill_bank:
                 return [(bank_tag(a[0], a[1]), 4, [(relu, a[0], a[1], a[2] + KP // a[0][2] - 2)])]
             if f == relu and a[2] == 0:

@@ -33,10 +33,10 @@ ALL_PASSES, FIRST_PASS, SECOND_PASS = (0, 1), (0,), (1,)
 W2_PIECES = tuple((g, c0, min(KP, 2 * L - c0)) for g in range(G2) for c0 in (0, KP))
 RUNS = KP // 8
 ORDER = ((4, 5, 0, 2, 1, 3), (4, 5, 0, 2, 3, 1))
-DEPTH = {"wraw": 6, "woven_w": 3, "woven_g": 1, "woven_v": 2, "woven_s": 2, "woven_x": 3, "res": 4,
+DEPTH = {"wraw": 6, "woven_w": 3, "woven_g": 1, "woven_v": 1, "woven_s": 3, "woven_x": 3, "res": 4,
          "state1": 4, "state2": 1, "wide2": 8, "wide4": 4, "obs2": 2, "obs4": 2}
 HIDDEN_DEPTH = {2 * QT: 2, QT: 3, P: 2}
-HEAD_RUNS = 44
+HEAD_RUNS = 34
 FRONT_A, FRONT_B = (0, 0, QT), (0, QT, QT)
 POOL_RUNS = 40
 
@@ -77,6 +77,7 @@ def tile_rssm_pa_kernel(tc, prev_state, prev_action, obs_bytes, obs_scale, eps,
         b2_rows = keep.tile([P, 2 * L], BF16)
         eps_sb = keep.tile([P, NT, L], BF16)
         ident = keep.tile([P, P], F32)
+        ident_bf = keep.tile([P, P], BF16)
 
         raw, woven, rows, obs, banks, hidden, result = {}, {}, {}, {}, {}, {}, {}
         copy = {"vector": nc.vector.tensor_copy, "scalar": nc.scalar.copy}
@@ -190,6 +191,22 @@ def tile_rssm_pa_kernel(tc, prev_state, prev_action, obs_bytes, obs_scale, eps,
             else:
                 copy[engine](out=woven[part][:].rearrange("p (s r e t) -> p r t e s", r=RUNS, e=2, t=4)[:, r0:r1],
                              in_=raw[half, g][:].rearrange("p t (r e s) -> p r t e s", e=2, s=4)[:, r0:r1, :, :, s0:s1])
+
+        def pass_w1(part, k):
+            half, g = part[:2]
+            banks[part, k] = psum.tile([P, 2 * P, 2, 2], BF16, name="tp")
+            cols = raw[half, g][:, :, 2 * P * k:2 * P * (k + 1)]
+            for u in range(2):
+                nc.tensor.matmul(banks[part, k][:, :, u, :], ident_bf[:], cols[:, 2 * u:2 * u + 2, :].rearrange("p e c -> p c e"),
+                                 start=True, stop=True)
+
+        def drain_w1(part, k):
+            if k == 0:
+                woven[part] = streamed(part[4], [P, WOVEN], BF16)
+            m0 = 2 * P * k // 4
+            out = woven[part][:].bitcast(F32).rearrange("p (s m w) -> p m s w", s=4, w=2)[:, m0:m0 + 2 * P // 4]
+            src = banks[part, k][:].rearrange("p c u e -> p (c u e)").bitcast(F32)
+            nc.scalar.copy(out=out, in_=src.rearrange("p (m s w) -> p m s w", s=4, w=2))
 
         def quant_w1(part):
             half, g, s0, s1, tag = part
@@ -332,10 +349,10 @@ def tile_rssm_pa_kernel(tc, prev_state, prev_action, obs_bytes, obs_scale, eps,
             return (half, g, 0, 4, "woven_w")
 
         def low(half, g):
-            return (half, g, 0, 3, "woven_g")
+            return (half, g, 0, 2, "woven_g")
 
         def high(half, g):
-            return (half, g, 3, 4, "woven_w")
+            return (half, g, 2, 4, "woven_w")
 
         def by(engine, part, r0=0, r1=RUNS):
             return (weave_w1, part, engine, r0, r1)
@@ -352,8 +369,8 @@ def tile_rssm_pa_kernel(tc, prev_state, prev_action, obs_bytes, obs_scale, eps,
             stores += [(store_std, n), (store_mean, n)] + ([(store_sample, n - 1)] if n else [])
         stores += [(store_sample,) + part for part in halves]
 
-        early, late = (0, 5, 0, 2, "woven_g"), (0, 5, 2, 4, "woven_w")
-        first, second = (0, 4, 0, 4, "woven_g"), (1, 5, 0, 4, "woven_g")
+        early = (0, 5, 0, 4, "woven_g")
+        first, second = (0, 4, 0, 4, "woven_w"), (1, 5, 0, 4, "woven_g")
         sync_q = [(load_obs, 0, 4), (load_w1, 0, 4), (load_scales,), (load_obs, 1, 4), (load_w1, 0, 5), (load_state, 0, 0), (load_state, 1, 0)]
         for q in GROUPS[0]:
             sync_q += [(load_obs, q, 2), (load_action, 2 * q), (load_action, 2 * q + 1)]
@@ -362,31 +379,31 @@ def tile_rssm_pa_kernel(tc, prev_state, prev_action, obs_bytes, obs_scale, eps,
         sync_q += [(load_w2, piece) for piece in W2_PIECES[1::-1] + W2_PIECES[2:]] + [(load_b2,), (load_eps,)] + stores
 
         tensor_q = [(turn, q, g) for q in GROUPS[0] for g in (4, 5)] + turns(front(0)) + [(turn, 0, 2), (front_pass, 0, 4, 0, 2), (turn, 1, 2), (front_pass, 0, 4, 2, 4)]
-        tensor_q += [(front_pass, 0, 5, 0, 2)] + turns(front(1)) + [(front_pass, 0, 5, 2, 4), (turn, 0, 3), (front_pass, 0, 0), (turn, 1, 3), (turn, 2, 4), (front_pass, 0, 2)]
+        tensor_q += [(front_pass, 0, 5, 0, 2)] + turns(front(1)) + [(front_pass, 0, 5, 2, 4), (turn, 0, 3), (turn, 1, 3), (front_pass, 0, 0), (turn, 2, 4), (front_pass, 0, 2)]
         tensor_q += [(turn, 2, 5), (front_pass, 0, 1)]
-        tensor_q += [(front_pass, 0, 3, 0, 2)] + turns((2, 2)) + [(front_pass, 0, 3, 2, 4)] + [(front_pass, 1, 4)] + turns((2, 0)) + [(front_pass, 1, 5, 0, 2), (turn, 3, 4), (front_pass, 1, 5, 2, 4), (turn, 3, 5)] + [(front_pass, 1, 0), (fill_bank, THIRD, 0, 0)]
+        tensor_q += [(front_pass, 0, 3, 0, 2)] + turns((2, 0)) + [(front_pass, 0, 3, 2, 4)] + turns((2, 2)) + [(pass_w1, whole(1, 0), 0), (pass_w1, whole(1, 0), 1), (front_pass, 1, 4)] + [(front_pass, 1, 5, 0, 2), (turn, 3, 4), (front_pass, 1, 5, 2, 4), (turn, 3, 5)] + [(front_pass, 1, 0), (fill_bank, THIRD, 0, 0)]
         tensor_q += [(front_pass, 1, 2), (front_pass, 1, 3), (front_pass, 1, 1), (fill_bank, THIRD, 0, 2)] + turns((3, 2))
         tensor_q += [(fill_bank, THIRD, 1, 0)] + turns((3, 0)) + [(fill_bank, THIRD, 1, 2), (heads, 0), (heads, 1)]
 
-        gpsimd_q = [by("gpsimd", early)] + [by("gpsimd", low(0, g), 0, POOL_RUNS) for g in (2, 3)] + [by("gpsimd", (1, 4, 0, 2, "woven_g")), by("gpsimd", low(1, 3), 0, POOL_RUNS)]
+        gpsimd_q = [by("gpsimd", low(0, g)) for g in (2, 3)] + [by("gpsimd", (1, 4, 0, 2, "woven_g")), by("gpsimd", low(1, 3))]
         gpsimd_q += [(weave_w2, W2_PIECES[1], "gpsimd"), (weave_h, FRONT_B, 0, "gpsimd")]
 
-        scalar_q = widens(0, 4) + [by("scalar", first, HEAD_RUNS)] + widens(1, 4) + [by("scalar", late)] + widens(0, 2) + [(drain, 0, 0)] + widens(1, 2) + [(drain, 1, 0)]
+        scalar_q = [(widen, 0, 4, "scalar"), by("scalar", first, HEAD_RUNS)] + widens(1, 4) + [by("scalar", early)] + widens(0, 2) + [(drain, 0, 0)] + widens(1, 2) + [(drain, 1, 0)]
         scalar_q += [by("scalar", whole(0, 0)), by("scalar", high(0, 2))] + empties(front(1)) + widens(2, 4)
         scalar_q += [by("scalar", whole(0, 1)), by("scalar", high(0, 3)), by("scalar", (1, 4, 2, 4, "woven_w"))] + widens(2, 2)
-        scalar_q += [(relu, FRONT, 0, 0), (widen, 6, 4, "scalar"), (relu, FRONT, 0, 2), (widen, 7, 4, "scalar")] + [by("scalar", whole(1, 0))] + empties((2, 0))
-        scalar_q += [by("scalar", whole(1, 2)), by("scalar", high(1, 3))] + widens(3, 2) + [(relu, THIRD, 0, 0)]
+        scalar_q += [(relu, FRONT, 0, 0)] + empties((2, 0)) + [(relu, FRONT, 0, 2), (widen, 6, 4, "scalar"), (drain_w1, whole(1, 0), 0), (widen, 7, 4, "scalar"), (drain_w1, whole(1, 0), 1)]
+        scalar_q += [by("scalar", whole(1, 2)), by("scalar", high(1, 3))] + widens(3, 2) + [(weave_h, FRONT_A, 0, "scalar"), (relu, THIRD, 0, 0)]
         scalar_q += [(weave_w2, W2_PIECES[0], "scalar"), (weave_w2, W2_PIECES[3], "scalar")] + relus(FRONT, 1) + [(relu, THIRD, 0, 2)]
         scalar_q += [(weave_h, FRONT_A, 1, "scalar")] + empties((3, 0)) + [(weave_h, FRONT_B, 1, "scalar")] + relus(THIRD, 1)
 
-        vector_q = [by("vector", first, 0, HEAD_RUNS), (product, 0, 4), (quant_w1, first), (product, 0, 5), (product, 1, 4), (product, 1, 5)]
-        vector_q += [(quant_x, front(4)), (quant_w1, late), (quant_w1, early), (quant_x, front(5))]
-        vector_q += empties(front(2)) + [(quant_x, front(0)), (quant_w1, whole(0, 0)), by("vector", low(0, 2), POOL_RUNS), (quant_w1, high(0, 2)), (quant_w1, low(0, 2)), (quant_x, front(2))]
-        vector_q += empties(front(3)) + [(quant_x, front(1)), (quant_w1, whole(0, 1)), by("vector", low(0, 3), POOL_RUNS), (quant_w1, high(0, 3)), (quant_w1, low(0, 3)), (quant_x, front(3))]
+        vector_q = [(widen, 1, 4, "vector"), by("vector", first, 0, HEAD_RUNS), (product, 0, 4), (quant_w1, first), (product, 0, 5), (product, 1, 4), (product, 1, 5)]
+        vector_q += [(quant_x, front(4)), (quant_w1, early), (quant_x, front(5))]
+        vector_q += empties(front(2)) + [(quant_x, front(0)), (quant_w1, whole(0, 0)), (quant_x, front(2)), (quant_w1, high(0, 2)), (quant_w1, low(0, 2))]
+        vector_q += empties(front(3)) + [(quant_x, front(1)), (quant_w1, whole(0, 1)), (quant_x, front(3)), (quant_w1, high(0, 3)), (quant_w1, low(0, 3))]
         vector_q += empties((2, 4)) + [(quant_w1, (1, 4, 2, 4, "woven_w")), (quant_w1, (1, 4, 0, 2, "woven_g")), by("vector", second), (quant_x, (2, 4)), (quant_w1, second)]
-        vector_q += empties((2, 2)) + [by("vector", low(1, 3), POOL_RUNS), (quant_w1, whole(1, 0)), (quant_x, (2, 2)), (quant_x, (2, 0)), by("vector", whole(1, 1))]
+        vector_q += empties((2, 2)) + [(quant_w1, whole(1, 0)), (quant_x, (2, 2)), (quant_x, (2, 0)), by("vector", whole(1, 1))]
         vector_q += [(quant_w1, whole(1, 2)), (quant_w1, high(1, 3)), (quant_w1, low(1, 3)), (quant_w1, whole(1, 1))]
-        vector_q += empties((3, 4)) + [(weave_h, FRONT_A, 0, "vector"), (quant_x, (3, 4)), (weave_w2, W2_PIECES[2], "vector")]
+        vector_q += empties((3, 4)) + [(weave_w2, W2_PIECES[2], "vector"), (quant_x, (3, 4))]
         vector_q += [(quant_h, FRONT_A, 0), (quant_w2, W2_PIECES[0]), (quant_w2, W2_PIECES[3]), (quant_w2, W2_PIECES[1]), (quant_w2, W2_PIECES[2])] + empties((3, 2))
         vector_q += [(quant_h, FRONT_A, 1), (quant_x, (3, 2)), (quant_x, (3, 0)), (quant_h, FRONT_B, 0)]
 
@@ -404,7 +421,7 @@ def tile_rssm_pa_kernel(tc, prev_state, prev_action, obs_bytes, obs_scale, eps,
         vector_q += [(f,) + part for f in (noise, shift) for part in halves]
         tensor_q += [(fill_bank, LAST, 0, 0), (heads, 2), (fill_bank, LAST, 0, 2), (heads, 3), (heads, 4), (fill_bank, LAST_A, 1, 0), (heads, 5)]
         tensor_q += [(fill_bank, LAST_B, 1, 0), (heads, NT - 2), (heads, NT - 1, FIRST_PASS), (heads, NT - 1, SECOND_PASS)]
-        behind = {by("gpsimd", low(1, 3), 0, POOL_RUNS): [(quant_w1, second)]}
+        behind = {by("gpsimd", low(0, 2)): [(quant_w1, early)], by("gpsimd", low(1, 3)): [(quant_w1, second)]}
 
         everything = sync_q + tensor_q + scalar_q + vector_q + gpsimd_q
         weaver = {step[1:-1]: step for step in everything if step[0] in (weave_w2, weave_h)}
@@ -429,10 +446,12 @@ def tile_rssm_pa_kernel(tc, prev_state, prev_action, obs_bytes, obs_scale, eps,
                 return [(turn,) + a, (load_scales,)]
             if f == quant_x:
                 return [emptier(*key) for key in banks_of(a[0])]
-            if f == weave_w1:
+            if f in (weave_w1, pass_w1):
                 return [(load_w1,) + a[0][:2]]
+            if f == drain_w1:
+                return [(pass_w1,) + a]
             if f == quant_w1:
-                return [step for step in everything if step[0] == weave_w1 and step[1] == a[0]]
+                return [step for step in everything if step[0] in (weave_w1, drain_w1) and step[1] == a[0]]
             if f == first_pass:
                 return w1_steps(quant_w1, 0, ORDER[0][0]) + [(quant_first,) + a]
             if f == quant_first:
@@ -466,7 +485,7 @@ def tile_rssm_pa_kernel(tc, prev_state, prev_action, obs_bytes, obs_scale, eps,
 
         def takes(f, *a):
             if f == load_w1:
-                return [("wraw", DEPTH["wraw"], w1_steps(weave_w1, *a))]
+                return [("wraw", DEPTH["wraw"], w1_steps(weave_w1, *a) + w1_steps(pass_w1, *a))]
             if f == load_w2:
                 return [("wraw", DEPTH["wraw"], [weaver[a]])]
             if f == load_obs:
@@ -480,6 +499,10 @@ def tile_rssm_pa_kernel(tc, prev_state, prev_action, obs_bytes, obs_scale, eps,
                 return [] if (n, g) in rows else [(tag, DEPTH[tag], [(turn, n // 2, g), (turn, n // 2, g + 1)])]
             if f == weave_w1:
                 return [] if a[0] in woven else [(a[0][4], DEPTH[a[0][4]], [(quant_w1, a[0])])]
+            if f == pass_w1:
+                return [("tp", 4, [(drain_w1,) + a])]
+            if f == drain_w1:
+                return [] if a[1] else [(a[0][4], DEPTH[a[0][4]], [(quant_w1, a[0])])]
             if f in (weave_w2, weave_h):
                 tag = weave_tag(a[-1])
                 return [(tag, DEPTH[tag], [(quant_w2 if f == weave_w2 else quant_h,) + a[:-1]])]
@@ -505,6 +528,7 @@ def tile_rssm_pa_kernel(tc, prev_state, prev_action, obs_bytes, obs_scale, eps,
 
         nc.vector.memset(ones[:], 1.0)
         make_identity(nc, ident[:])
+        make_identity(nc, ident_bf[:])
         nc.scalar.activation(scale_mixed[:ACTION_ROWS, :], ones[:], ACT.Sqrt)
 
         done, held = set(), {}

@@ -34,7 +34,7 @@ W2_PIECES = tuple((g, c0, min(KP, 2 * L - c0)) for g in range(G2) for c0 in (0, 
 RUNS = KP // 8
 ORDER = ((4, 5, 0, 2, 1, 3), (4, 5, 0, 2, 3, 1))
 DEPTH = {"wraw": 6, "woven_w": 3, "woven_g": 1, "woven_v": 1, "woven_s": 3, "woven_x": 3, "res": 4,
-         "state1": 4, "state2": 1, "wide2": 8, "wide4": 4, "obs2": 2, "obs4": 2}
+         "state1": 4, "state2": 1, "wide2": 8, "wide4": 2, "obs2": 2, "obs4": 2}
 HIDDEN_DEPTH = {2 * QT: 2, QT: 3, P: 2}
 HEAD_RUNS = 34
 FRONT_A, FRONT_B = (0, 0, QT), (0, QT, QT)
@@ -120,9 +120,13 @@ def tile_rssm_pa_kernel(tc, prev_state, prev_action, obs_bytes, obs_scale, eps,
 
         def wide_tile(n, g):
             if (n, g) not in rows:
-                buf = streamed("wide%d" % g, [P, 2 * KP], BF16)
-                rows[n, g, "tile"] = buf
-                rows[n, g], rows[n, g + 1] = buf[:, :KP], buf[:, KP:]
+                tiles = 1 if g == STATE_PASSES else 2
+                buf = streamed("wide%d" % g, [P, tiles * 2 * KP], BF16)
+                rows[n, g, "all"] = buf[:]
+                for i in range(tiles):
+                    part = buf[:, 2 * KP * i:2 * KP * (i + 1)]
+                    rows[n + i, g, "tile"] = part
+                    rows[n + i, g], rows[n + i, g + 1] = part[:, :KP], part[:, KP:]
             return rows[n, g, "tile"]
 
         def load_action(n):
@@ -140,6 +144,10 @@ def tile_rssm_pa_kernel(tc, prev_state, prev_action, obs_bytes, obs_scale, eps,
         def widen(n, g, engine):
             c0, c1 = obs_cols(g)
             copy[engine](out=wide_tile(n, g)[:, 2 * KP - (c1 - c0):], in_=obs[n // 2, g][:, n % 2, :].bitcast(FP8))
+
+        def widen_both(q, g):
+            wide_tile(2 * q, g)
+            nc.scalar.copy(out=rows[2 * q, g, "all"], in_=obs[q, g][:].rearrange("p i c -> p (i c)").bitcast(FP8))
 
         def turn(q, g):
             banks[q, g] = psum.tile([P, 2, QT], F32, name=turn_tag(q, g))
@@ -253,6 +261,11 @@ def tile_rssm_pa_kernel(tc, prev_state, prev_action, obs_bytes, obs_scale, eps,
                     acc = psum.tile([P, KP], F32, name="acc")
                     banks[FRONT, 0, t] = acc[:]
                 mm1((0, QT * q, QT), 0, t, ORDER[0][0])
+
+        def warm_up(k):
+            idle = psum.tile([P, P], F32, name="acc")
+            for j in range(2):
+                nc.tensor.matmul(idle[:], ident[:], ident[:], start=True, stop=True)
 
         def bank_start(span, t):
             return t - t % (KP // span[2])
@@ -369,35 +382,34 @@ def tile_rssm_pa_kernel(tc, prev_state, prev_action, obs_bytes, obs_scale, eps,
             stores += [(store_std, n), (store_mean, n)] + ([(store_sample, n - 1)] if n else [])
         stores += [(store_sample,) + part for part in halves]
 
-        early = (0, 5, 0, 4, "woven_g")
-        first, second = (0, 4, 0, 4, "woven_w"), (1, 5, 0, 4, "woven_g")
-        sync_q = [(load_obs, 0, 4), (load_w1, 0, 4), (load_scales,), (load_obs, 1, 4), (load_w1, 0, 5), (load_state, 0, 0), (load_state, 1, 0)]
-        for q in GROUPS[0]:
-            sync_q += [(load_obs, q, 2), (load_action, 2 * q), (load_action, 2 * q + 1)]
+        early, late = low(0, 5), high(0, 5)
+        first, second = (0, 4, 0, 4, "woven_g"), (1, 5, 0, 4, "woven_g")
+        sync_q = [(load_obs, 0, 4), (load_w1, 0, 4), (load_scales,), (load_obs, 1, 4), (load_w1, 0, 5), (load_obs, 0, 2), (load_state, 0, 0), (load_state, 1, 0)]
+        sync_q += [(load_obs, 1, 2)] + [(load_action, n) for n in range(4)]
         sync_q += [(load_w1, 0, 0), (load_w1, 0, 2), (load_state, 0, 1), (load_state, 1, 1), (load_obs, 2, 4), (load_w1, 0, 1), (load_w1, 0, 3), (load_b1,)]
         sync_q += rows_of(2)[1:] + [(load_w1, 1, g) for g in (4, 5, 0)] + [(load_obs, 3, 4)] + [(load_w1, 1, g) for g in (3, 1, 2)] + rows_of(3)[1:]
         sync_q += [(load_w2, piece) for piece in W2_PIECES[1::-1] + W2_PIECES[2:]] + [(load_b2,), (load_eps,)] + stores
 
         tensor_q = [(turn, q, g) for q in GROUPS[0] for g in (4, 5)] + turns(front(0)) + [(turn, 0, 2), (front_pass, 0, 4, 0, 2), (turn, 1, 2), (front_pass, 0, 4, 2, 4)]
-        tensor_q += [(front_pass, 0, 5, 0, 2)] + turns(front(1)) + [(front_pass, 0, 5, 2, 4), (turn, 0, 3), (turn, 1, 3), (front_pass, 0, 0), (turn, 2, 4), (front_pass, 0, 2)]
+        tensor_q += [(front_pass, 0, 5, 0, 2)] + turns(front(1)) + [(turn, 0, 3), (front_pass, 0, 5, 2, 4), (turn, 1, 3), (front_pass, 0, 0), (turn, 2, 4), (front_pass, 0, 2)]
         tensor_q += [(turn, 2, 5), (front_pass, 0, 1)]
         tensor_q += [(front_pass, 0, 3, 0, 2)] + turns((2, 0)) + [(front_pass, 0, 3, 2, 4)] + turns((2, 2)) + [(pass_w1, whole(1, 0), 0), (pass_w1, whole(1, 0), 1), (front_pass, 1, 4)] + [(front_pass, 1, 5, 0, 2), (turn, 3, 4), (front_pass, 1, 5, 2, 4), (turn, 3, 5)] + [(front_pass, 1, 0), (fill_bank, THIRD, 0, 0)]
         tensor_q += [(front_pass, 1, 2), (front_pass, 1, 3), (front_pass, 1, 1), (fill_bank, THIRD, 0, 2)] + turns((3, 2))
         tensor_q += [(fill_bank, THIRD, 1, 0)] + turns((3, 0)) + [(fill_bank, THIRD, 1, 2), (heads, 0), (heads, 1)]
 
-        gpsimd_q = [by("gpsimd", low(0, g)) for g in (2, 3)] + [by("gpsimd", (1, 4, 0, 2, "woven_g")), by("gpsimd", low(1, 3))]
+        gpsimd_q = [by("gpsimd", early)] + [by("gpsimd", low(0, g)) for g in (2, 3)] + [by("gpsimd", (1, 4, 0, 2, "woven_g")), by("gpsimd", low(1, 3))]
         gpsimd_q += [(weave_w2, W2_PIECES[1], "gpsimd"), (weave_h, FRONT_B, 0, "gpsimd")]
 
-        scalar_q = [(widen, 0, 4, "scalar"), by("scalar", first, HEAD_RUNS)] + widens(1, 4) + [by("scalar", early)] + widens(0, 2) + [(drain, 0, 0)] + widens(1, 2) + [(drain, 1, 0)]
-        scalar_q += [by("scalar", whole(0, 0)), by("scalar", high(0, 2))] + empties(front(1)) + widens(2, 4)
+        scalar_q = [(widen, 0, 4, "scalar"), by("scalar", first, HEAD_RUNS)] + widens(1, 4) + [by("scalar", late)] + widens(0, 2) + [(drain, 0, 0)] + widens(1, 2) + [(drain, 1, 0)]
+        scalar_q += [by("scalar", whole(0, 0)), by("scalar", high(0, 2))] + empties(front(1)) + [(widen_both, 2, 4)]
         scalar_q += [by("scalar", whole(0, 1)), by("scalar", high(0, 3)), by("scalar", (1, 4, 2, 4, "woven_w"))] + widens(2, 2)
-        scalar_q += [(relu, FRONT, 0, 0)] + empties((2, 0)) + [(relu, FRONT, 0, 2), (widen, 6, 4, "scalar"), (drain_w1, whole(1, 0), 0), (widen, 7, 4, "scalar"), (drain_w1, whole(1, 0), 1)]
+        scalar_q += [(relu, FRONT, 0, 0)] + empties((2, 0)) + [(relu, FRONT, 0, 2), (widen_both, 3, 4), (drain_w1, whole(1, 0), 0), (drain_w1, whole(1, 0), 1)]
         scalar_q += [by("scalar", whole(1, 2)), by("scalar", high(1, 3))] + widens(3, 2) + [(weave_h, FRONT_A, 0, "scalar"), (relu, THIRD, 0, 0)]
         scalar_q += [(weave_w2, W2_PIECES[0], "scalar"), (weave_w2, W2_PIECES[3], "scalar")] + relus(FRONT, 1) + [(relu, THIRD, 0, 2)]
         scalar_q += [(weave_h, FRONT_A, 1, "scalar")] + empties((3, 0)) + [(weave_h, FRONT_B, 1, "scalar")] + relus(THIRD, 1)
 
         vector_q = [(widen, 1, 4, "vector"), by("vector", first, 0, HEAD_RUNS), (product, 0, 4), (quant_w1, first), (product, 0, 5), (product, 1, 4), (product, 1, 5)]
-        vector_q += [(quant_x, front(4)), (quant_w1, early), (quant_x, front(5))]
+        vector_q += [(quant_x, front(4)), (quant_w1, late), (quant_w1, early), (quant_x, front(5))]
         vector_q += empties(front(2)) + [(quant_x, front(0)), (quant_w1, whole(0, 0)), (quant_x, front(2)), (quant_w1, high(0, 2)), (quant_w1, low(0, 2))]
         vector_q += empties(front(3)) + [(quant_x, front(1)), (quant_w1, whole(0, 1)), (quant_x, front(3)), (quant_w1, high(0, 3)), (quant_w1, low(0, 3))]
         vector_q += empties((2, 4)) + [(quant_w1, (1, 4, 2, 4, "woven_w")), (quant_w1, (1, 4, 0, 2, "woven_g")), by("vector", second), (quant_x, (2, 4)), (quant_w1, second)]
@@ -421,11 +433,13 @@ def tile_rssm_pa_kernel(tc, prev_state, prev_action, obs_bytes, obs_scale, eps,
         vector_q += [(f,) + part for f in (noise, shift) for part in halves]
         tensor_q += [(fill_bank, LAST, 0, 0), (heads, 2), (fill_bank, LAST, 0, 2), (heads, 3), (heads, 4), (fill_bank, LAST_A, 1, 0), (heads, 5)]
         tensor_q += [(fill_bank, LAST_B, 1, 0), (heads, NT - 2), (heads, NT - 1, FIRST_PASS), (heads, NT - 1, SECOND_PASS)]
-        behind = {by("gpsimd", low(0, 2)): [(quant_w1, early)], by("gpsimd", low(1, 3)): [(quant_w1, second)]}
+        behind = {(widen, 1, 4, "vector"): [(widen, 0, 4, "scalar")], by("gpsimd", low(1, 3)): [(quant_w1, second)]}
 
         everything = sync_q + tensor_q + scalar_q + vector_q + gpsimd_q
         weaver = {step[1:-1]: step for step in everything if step[0] in (weave_w2, weave_h)}
         widener = {step[1:-1]: step for step in everything if step[0] == widen}
+
+        widener.update({(2 * step[1] + i, step[2]): step for step in everything if step[0] == widen_both for i in range(2)})
 
         def w1_steps(f, half, g):
             return [step for step in everything if step[0] == f and step[1][:2] == (half, g)]
@@ -436,6 +450,8 @@ def tile_rssm_pa_kernel(tc, prev_state, prev_action, obs_bytes, obs_scale, eps,
         def needs(f, *a):
             if f == widen:
                 return [(load_obs, a[0] // 2, a[1])]
+            if f == widen_both:
+                return [(load_obs,) + a]
             if f == turn:
                 q, g = a
                 if g < STATE_PASSES:
@@ -493,6 +509,8 @@ def tile_rssm_pa_kernel(tc, prev_state, prev_action, obs_bytes, obs_scale, eps,
             if f == load_state:
                 n = 1 if a[0] in GROUPS[0] else STATE_PASSES
                 return [("state%d" % n, DEPTH["state%d" % n], [(turn, a[0], a[1] + j) for j in range(n)])]
+            if f == widen_both:
+                return [("wide4", DEPTH["wide4"], [(turn, a[0], 4), (turn, a[0], 5)])]
             if f in (load_action, widen):
                 n, g = a[0], a[1] if f == widen else STATE_PASSES
                 tag = "wide%d" % g

@@ -38,7 +38,7 @@ DEPTH = {"wraw": 6, "woven_w": 3, "woven_g": 1, "woven_v": 1, "woven_s": 3, "wov
 HIDDEN_DEPTH = {2 * QT: 2, QT: 3, P: 2}
 HEAD_RUNS = 34
 FRONT_A, FRONT_B = (0, 0, QT), (0, QT, QT)
-POOL_RUNS = 40
+POOL_RUNS = 32
 
 
 def tile_rssm_pa_kernel(tc, prev_state, prev_action, obs_bytes, obs_scale, eps,
@@ -382,7 +382,9 @@ def tile_rssm_pa_kernel(tc, prev_state, prev_action, obs_bytes, obs_scale, eps,
             stores += [(store_std, n), (store_mean, n)] + ([(store_sample, n - 1)] if n else [])
         stores += [(store_sample,) + part for part in halves]
 
-        early, late = low(0, 5), high(0, 5)
+        def shared(half, g):
+            return (half, g, 0, 4, "woven_g")
+
         first, second = (0, 4, 0, 4, "woven_g"), (1, 5, 0, 4, "woven_g")
         sync_q = [(load_obs, 0, 4), (load_w1, 0, 4), (load_scales,), (load_obs, 1, 4), (load_w1, 0, 5), (load_obs, 0, 2), (load_state, 0, 0), (load_state, 1, 0)]
         sync_q += [(load_obs, 1, 2)] + [(load_action, n) for n in range(4)]
@@ -390,31 +392,32 @@ def tile_rssm_pa_kernel(tc, prev_state, prev_action, obs_bytes, obs_scale, eps,
         sync_q += rows_of(2)[1:] + [(load_w1, 1, g) for g in (4, 5, 0)] + [(load_obs, 3, 4)] + [(load_w1, 1, g) for g in (3, 1, 2)] + rows_of(3)[1:]
         sync_q += [(load_w2, piece) for piece in W2_PIECES[1::-1] + W2_PIECES[2:]] + [(load_b2,), (load_eps,)] + stores
 
-        tensor_q = [(turn, q, g) for q in GROUPS[0] for g in (4, 5)] + turns(front(0)) + [(turn, 0, 2), (front_pass, 0, 4, 0, 2), (turn, 1, 2), (front_pass, 0, 4, 2, 4)]
-        tensor_q += [(front_pass, 0, 5, 0, 2)] + turns(front(1)) + [(turn, 0, 3), (front_pass, 0, 5, 2, 4), (turn, 1, 3), (front_pass, 0, 0), (turn, 2, 4), (front_pass, 0, 2)]
-        tensor_q += [(turn, 2, 5), (front_pass, 0, 1)]
-        tensor_q += [(front_pass, 0, 3, 0, 2)] + turns((2, 0)) + [(front_pass, 0, 3, 2, 4)] + turns((2, 2)) + [(pass_w1, whole(1, 0), 0), (pass_w1, whole(1, 0), 1), (front_pass, 1, 4)] + [(front_pass, 1, 5, 0, 2), (turn, 3, 4), (front_pass, 1, 5, 2, 4), (turn, 3, 5)] + [(front_pass, 1, 0), (fill_bank, THIRD, 0, 0)]
+        tensor_q = [(turn, q, g) for q in GROUPS[0] for g in (4, 5)] + turns(front(0)) + turns(front(2)) + [(front_pass, 0, 4)]
+        tensor_q += [(front_pass, 0, 5, 0, 2)] + turns(front(1)) + [(front_pass, 0, 5, 2, 4)] + turns(front(3))
+        tensor_q += [(front_pass, 0, 0)] + turns((2, 4)) + [(front_pass, 0, 2), (front_pass, 0, 1), (front_pass, 0, 3)] + turns((2, 0))
+        tensor_q += [(pass_w1, whole(1, 0), 0), (pass_w1, whole(1, 0), 1)] + turns((2, 2)) + [(front_pass, 1, 4), (front_pass, 1, 5)]
+        tensor_q += turns((3, 4)) + [(front_pass, 1, 0), (fill_bank, THIRD, 0, 0)]
         tensor_q += [(front_pass, 1, 2), (front_pass, 1, 3), (front_pass, 1, 1), (fill_bank, THIRD, 0, 2)] + turns((3, 2))
         tensor_q += [(fill_bank, THIRD, 1, 0)] + turns((3, 0)) + [(fill_bank, THIRD, 1, 2), (heads, 0), (heads, 1)]
 
-        gpsimd_q = [by("gpsimd", early)] + [by("gpsimd", low(0, g)) for g in (2, 3)] + [by("gpsimd", (1, 4, 0, 2, "woven_g")), by("gpsimd", low(1, 3))]
+        gpsimd_q = [by("gpsimd", shared(*key), 0, POOL_RUNS) for key in ((0, 5), (0, 2), (0, 3), (1, 4), (1, 3))]
         gpsimd_q += [(weave_w2, W2_PIECES[1], "gpsimd"), (weave_h, FRONT_B, 0, "gpsimd")]
 
-        scalar_q = [(widen, 0, 4, "scalar"), by("scalar", first, HEAD_RUNS)] + widens(1, 4) + [by("scalar", late)] + widens(0, 2) + [(drain, 0, 0)] + widens(1, 2) + [(drain, 1, 0)]
-        scalar_q += [by("scalar", whole(0, 0)), by("scalar", high(0, 2))] + empties(front(1)) + [(widen_both, 2, 4)]
-        scalar_q += [by("scalar", whole(0, 1)), by("scalar", high(0, 3)), by("scalar", (1, 4, 2, 4, "woven_w"))] + widens(2, 2)
-        scalar_q += [(relu, FRONT, 0, 0)] + empties((2, 0)) + [(relu, FRONT, 0, 2), (widen_both, 3, 4), (drain_w1, whole(1, 0), 0), (drain_w1, whole(1, 0), 1)]
-        scalar_q += [by("scalar", whole(1, 2)), by("scalar", high(1, 3))] + widens(3, 2) + [(weave_h, FRONT_A, 0, "scalar"), (relu, THIRD, 0, 0)]
+        scalar_q = [(widen, 0, 4, "scalar"), by("scalar", first, HEAD_RUNS)] + widens(1, 4) + [by("scalar", shared(0, 5), POOL_RUNS)] + widens(0, 2) + [(drain, 0, 0)] + widens(1, 2) + [(drain, 1, 0)]
+        scalar_q += [by("scalar", whole(0, 0)), by("scalar", shared(0, 2), POOL_RUNS)] + empties(front(1)) + [(widen_both, 2, 4)]
+        scalar_q += [by("scalar", whole(0, 1)), by("scalar", shared(0, 3), POOL_RUNS)] + widens(2, 2) + [by("scalar", shared(1, 4), POOL_RUNS)]
+        scalar_q += [(relu, FRONT, 0, 0)] + empties((2, 0)) + [(relu, FRONT, 0, 2), (drain_w1, whole(1, 0), 0), (drain_w1, whole(1, 0), 1), (widen_both, 3, 4)]
+        scalar_q += [by("scalar", whole(1, 2)), by("scalar", shared(1, 3), POOL_RUNS)] + widens(3, 2) + [(weave_h, FRONT_A, 0, "scalar"), (relu, THIRD, 0, 0)]
         scalar_q += [(weave_w2, W2_PIECES[0], "scalar"), (weave_w2, W2_PIECES[3], "scalar")] + relus(FRONT, 1) + [(relu, THIRD, 0, 2)]
         scalar_q += [(weave_h, FRONT_A, 1, "scalar")] + empties((3, 0)) + [(weave_h, FRONT_B, 1, "scalar")] + relus(THIRD, 1)
 
         vector_q = [(widen, 1, 4, "vector"), by("vector", first, 0, HEAD_RUNS), (product, 0, 4), (quant_w1, first), (product, 0, 5), (product, 1, 4), (product, 1, 5)]
-        vector_q += [(quant_x, front(4)), (quant_w1, late), (quant_w1, early), (quant_x, front(5))]
-        vector_q += empties(front(2)) + [(quant_x, front(0)), (quant_w1, whole(0, 0)), (quant_x, front(2)), (quant_w1, high(0, 2)), (quant_w1, low(0, 2))]
-        vector_q += empties(front(3)) + [(quant_x, front(1)), (quant_w1, whole(0, 1)), (quant_x, front(3)), (quant_w1, high(0, 3)), (quant_w1, low(0, 3))]
-        vector_q += empties((2, 4)) + [(quant_w1, (1, 4, 2, 4, "woven_w")), (quant_w1, (1, 4, 0, 2, "woven_g")), by("vector", second), (quant_x, (2, 4)), (quant_w1, second)]
+        vector_q += [(quant_x, front(4)), (quant_w1, shared(0, 5)), (quant_x, front(5))]
+        vector_q += empties(front(2)) + [(quant_x, front(0)), (quant_w1, whole(0, 0)), (quant_x, front(2)), (quant_w1, shared(0, 2))]
+        vector_q += empties(front(3)) + [(quant_x, front(1)), (quant_w1, whole(0, 1)), (quant_x, front(3)), (quant_w1, shared(0, 3))]
+        vector_q += empties((2, 4)) + [(quant_w1, shared(1, 4)), by("vector", second), (quant_x, (2, 4)), (quant_w1, second)]
         vector_q += empties((2, 2)) + [(quant_w1, whole(1, 0)), (quant_x, (2, 2)), (quant_x, (2, 0)), by("vector", whole(1, 1))]
-        vector_q += [(quant_w1, whole(1, 2)), (quant_w1, high(1, 3)), (quant_w1, low(1, 3)), (quant_w1, whole(1, 1))]
+        vector_q += [(quant_w1, whole(1, 2)), (quant_w1, shared(1, 3)), (quant_w1, whole(1, 1))]
         vector_q += empties((3, 4)) + [(weave_w2, W2_PIECES[2], "vector"), (quant_x, (3, 4))]
         vector_q += [(quant_h, FRONT_A, 0), (quant_w2, W2_PIECES[0]), (quant_w2, W2_PIECES[3]), (quant_w2, W2_PIECES[1]), (quant_w2, W2_PIECES[2])] + empties((3, 2))
         vector_q += [(quant_h, FRONT_A, 1), (quant_x, (3, 2)), (quant_x, (3, 0)), (quant_h, FRONT_B, 0)]
@@ -433,7 +436,7 @@ def tile_rssm_pa_kernel(tc, prev_state, prev_action, obs_bytes, obs_scale, eps,
         vector_q += [(f,) + part for f in (noise, shift) for part in halves]
         tensor_q += [(fill_bank, LAST, 0, 0), (heads, 2), (fill_bank, LAST, 0, 2), (heads, 3), (heads, 4), (fill_bank, LAST_A, 1, 0), (heads, 5)]
         tensor_q += [(fill_bank, LAST_B, 1, 0), (heads, NT - 2), (heads, NT - 1, FIRST_PASS), (heads, NT - 1, SECOND_PASS)]
-        behind = {(widen, 1, 4, "vector"): [(widen, 0, 4, "scalar")], by("gpsimd", low(1, 3)): [(quant_w1, second)]}
+        behind = {(widen, 1, 4, "vector"): [(widen, 0, 4, "scalar")], by("gpsimd", shared(1, 3), 0, POOL_RUNS): [(quant_w1, second)], by("scalar", shared(1, 3), POOL_RUNS): [(quant_w1, second)]}
 
         everything = sync_q + tensor_q + scalar_q + vector_q + gpsimd_q
         weaver = {step[1:-1]: step for step in everything if step[0] in (weave_w2, weave_h)}

@@ -38,7 +38,8 @@ DEPTH = {"wraw": 6, "woven_w": 3, "woven_g": 1, "woven_v": 1, "woven_s": 3, "wov
 HIDDEN_DEPTH = {2 * QT: 2, QT: 3, P: 2}
 HEAD_RUNS = 34
 FRONT_A, FRONT_B = (0, 0, QT), (0, QT, QT)
-POOL_RUNS = 32
+POOL_RUNS = 40
+LATE_RUNS = 44
 
 
 def tile_rssm_pa_kernel(tc, prev_state, prev_action, obs_bytes, obs_scale, eps,
@@ -263,9 +264,9 @@ def tile_rssm_pa_kernel(tc, prev_state, prev_action, obs_bytes, obs_scale, eps,
                 mm1((0, QT * q, QT), 0, t, ORDER[0][0])
 
         def warm_up(k):
-            idle = psum.tile([P, P], F32, name="acc")
+            idle = psum.tile([P, KP], F32, name="acc")
             for j in range(2):
-                nc.tensor.matmul(idle[:], ident[:], ident[:], start=True, stop=True)
+                nc.tensor.matmul(idle[:], ident_bf[:], rows[0, ORDER[0][0]], start=True, stop=True)
 
         def bank_start(span, t):
             return t - t % (KP // span[2])
@@ -379,7 +380,8 @@ def tile_rssm_pa_kernel(tc, prev_state, prev_action, obs_bytes, obs_scale, eps,
         halves = [(NT - 1, 0, L // 2), (NT - 1, L // 2, L)]
         stores = []
         for n in range(NT):
-            stores += [(store_std, n), (store_mean, n)] + ([(store_sample, n - 1)] if n else [])
+            before = [(store_sample, n - 1)] if n else []
+            stores += [(store_std, n)] + (before + [(store_mean, n)] if n >= NT - 2 else [(store_mean, n)] + before)
         stores += [(store_sample,) + part for part in halves]
 
         def shared(half, g):
@@ -389,7 +391,7 @@ def tile_rssm_pa_kernel(tc, prev_state, prev_action, obs_bytes, obs_scale, eps,
         sync_q = [(load_obs, 0, 4), (load_w1, 0, 4), (load_scales,), (load_obs, 1, 4), (load_w1, 0, 5), (load_obs, 0, 2), (load_state, 0, 0), (load_state, 1, 0)]
         sync_q += [(load_obs, 1, 2)] + [(load_action, n) for n in range(4)]
         sync_q += [(load_w1, 0, 0), (load_w1, 0, 2), (load_state, 0, 1), (load_state, 1, 1), (load_obs, 2, 4), (load_w1, 0, 1), (load_w1, 0, 3), (load_b1,)]
-        sync_q += rows_of(2)[1:] + [(load_w1, 1, g) for g in (4, 5, 0)] + [(load_obs, 3, 4)] + [(load_w1, 1, g) for g in (3, 1, 2)] + rows_of(3)[1:]
+        sync_q += [(load_w1, 1, 4)] + rows_of(2)[2:] + [(load_state, 2, 0)] + [(load_w1, 1, g) for g in (5, 0)] + [(load_obs, 3, 4)] + [(load_w1, 1, g) for g in (3, 1, 2)] + rows_of(3)[1:]
         sync_q += [(load_w2, piece) for piece in W2_PIECES[1::-1] + W2_PIECES[2:]] + [(load_b2,), (load_eps,)] + stores
 
         tensor_q = [(turn, q, g) for q in GROUPS[0] for g in (4, 5)] + turns(front(0)) + turns(front(2)) + [(front_pass, 0, 4)]
@@ -400,12 +402,12 @@ def tile_rssm_pa_kernel(tc, prev_state, prev_action, obs_bytes, obs_scale, eps,
         tensor_q += [(front_pass, 1, 2), (front_pass, 1, 3), (front_pass, 1, 1), (fill_bank, THIRD, 0, 2)] + turns((3, 2))
         tensor_q += [(fill_bank, THIRD, 1, 0)] + turns((3, 0)) + [(fill_bank, THIRD, 1, 2), (heads, 0), (heads, 1)]
 
-        gpsimd_q = [by("gpsimd", shared(*key), 0, POOL_RUNS) for key in ((0, 5), (0, 2), (0, 3), (1, 4), (1, 3))]
+        gpsimd_q = [by("gpsimd", shared(*key), 0, POOL_RUNS) for key in ((0, 5), (0, 2), (0, 3), (1, 5), (1, 3))]
         gpsimd_q += [(weave_w2, W2_PIECES[1], "gpsimd"), (weave_h, FRONT_B, 0, "gpsimd")]
 
         scalar_q = [(widen, 0, 4, "scalar"), by("scalar", first, HEAD_RUNS)] + widens(1, 4) + [by("scalar", shared(0, 5), POOL_RUNS)] + widens(0, 2) + [(drain, 0, 0)] + widens(1, 2) + [(drain, 1, 0)]
         scalar_q += [by("scalar", whole(0, 0)), by("scalar", shared(0, 2), POOL_RUNS)] + empties(front(1)) + [(widen_both, 2, 4)]
-        scalar_q += [by("scalar", whole(0, 1)), by("scalar", shared(0, 3), POOL_RUNS)] + widens(2, 2) + [by("scalar", shared(1, 4), POOL_RUNS)]
+        scalar_q += [by("scalar", whole(0, 1)), by("scalar", shared(0, 3), POOL_RUNS), by("scalar", whole(1, 4), LATE_RUNS)] + widens(2, 2) + [by("scalar", shared(1, 5), POOL_RUNS)]
         scalar_q += [(relu, FRONT, 0, 0)] + empties((2, 0)) + [(relu, FRONT, 0, 2), (drain_w1, whole(1, 0), 0), (drain_w1, whole(1, 0), 1), (widen_both, 3, 4)]
         scalar_q += [by("scalar", whole(1, 2)), by("scalar", shared(1, 3), POOL_RUNS)] + widens(3, 2) + [(weave_h, FRONT_A, 0, "scalar"), (relu, THIRD, 0, 0)]
         scalar_q += [(weave_w2, W2_PIECES[0], "scalar"), (weave_w2, W2_PIECES[3], "scalar")] + relus(FRONT, 1) + [(relu, THIRD, 0, 2)]
@@ -415,7 +417,7 @@ def tile_rssm_pa_kernel(tc, prev_state, prev_action, obs_bytes, obs_scale, eps,
         vector_q += [(quant_x, front(4)), (quant_w1, shared(0, 5)), (quant_x, front(5))]
         vector_q += empties(front(2)) + [(quant_x, front(0)), (quant_w1, whole(0, 0)), (quant_x, front(2)), (quant_w1, shared(0, 2))]
         vector_q += empties(front(3)) + [(quant_x, front(1)), (quant_w1, whole(0, 1)), (quant_x, front(3)), (quant_w1, shared(0, 3))]
-        vector_q += empties((2, 4)) + [(quant_w1, shared(1, 4)), by("vector", second), (quant_x, (2, 4)), (quant_w1, second)]
+        vector_q += empties((2, 4)) + [by("vector", whole(1, 4), 0, LATE_RUNS), (quant_x, (2, 4)), (quant_w1, whole(1, 4)), (quant_w1, shared(1, 5))]
         vector_q += empties((2, 2)) + [(quant_w1, whole(1, 0)), (quant_x, (2, 2)), (quant_x, (2, 0)), by("vector", whole(1, 1))]
         vector_q += [(quant_w1, whole(1, 2)), (quant_w1, shared(1, 3)), (quant_w1, whole(1, 1))]
         vector_q += empties((3, 4)) + [(weave_w2, W2_PIECES[2], "vector"), (quant_x, (3, 4))]
@@ -431,12 +433,12 @@ def tile_rssm_pa_kernel(tc, prev_state, prev_action, obs_bytes, obs_scale, eps,
         for n in range(NT - 3):
             vector_q += [(bias_wide, n)] + ([(noise, n - 1)] if n else []) + [(bias_narrow, n)]
             vector_q += ([(shift, n - 1)] if n else []) + after_tile[n]
-        vector_q += [(bias_wide, 5), (noise, 4), (bias_narrow, 5), (shift, 4), (quant_h, LAST_A, 1), (noise, 5), (weave_h, LAST_B, 1, "vector"), (bias_wide, 6), (quant_h, LAST_B, 1)]
-        vector_q += [(shift, 5), (bias_narrow, 6), (bias_wide, 7), (noise, 6), (bias_narrow, 7), (shift, 6)]
+        vector_q += [(bias_wide, 5), (noise, 4), (bias_narrow, 5), (shift, 4), (quant_h, LAST_A, 1), (noise, 5), (bias_wide, 6), (weave_h, LAST_B, 1, "vector"), (shift, 5), (quant_h, LAST_B, 1)]
+        vector_q += [(bias_narrow, 6), (noise, 6), (bias_wide, 7), (shift, 6), (bias_narrow, 7)]
         vector_q += [(f,) + part for f in (noise, shift) for part in halves]
         tensor_q += [(fill_bank, LAST, 0, 0), (heads, 2), (fill_bank, LAST, 0, 2), (heads, 3), (heads, 4), (fill_bank, LAST_A, 1, 0), (heads, 5)]
         tensor_q += [(fill_bank, LAST_B, 1, 0), (heads, NT - 2), (heads, NT - 1, FIRST_PASS), (heads, NT - 1, SECOND_PASS)]
-        behind = {(widen, 1, 4, "vector"): [(widen, 0, 4, "scalar")], by("gpsimd", shared(1, 3), 0, POOL_RUNS): [(quant_w1, second)], by("scalar", shared(1, 3), POOL_RUNS): [(quant_w1, second)]}
+        behind = {(widen, 1, 4, "vector"): [(widen, 0, 4, "scalar")]}
 
         everything = sync_q + tensor_q + scalar_q + vector_q + gpsimd_q
         weaver = {step[1:-1]: step for step in everything if step[0] in (weave_w2, weave_h)}

@@ -38,8 +38,7 @@ DEPTH = {"wraw": 6, "woven_w": 3, "woven_g": 1, "woven_v": 1, "woven_s": 3, "wov
 HIDDEN_DEPTH = {2 * QT: 2, QT: 3, P: 2}
 HEAD_RUNS = 34
 FRONT_A, FRONT_B = (0, 0, QT), (0, QT, QT)
-POOL_RUNS = 40
-LATE_RUNS = 44
+POOL_RUNS = 48
 
 
 def tile_rssm_pa_kernel(tc, prev_state, prev_action, obs_bytes, obs_scale, eps,
@@ -394,21 +393,21 @@ def tile_rssm_pa_kernel(tc, prev_state, prev_action, obs_bytes, obs_scale, eps,
         sync_q += [(load_w1, 1, 4)] + rows_of(2)[2:] + [(load_state, 2, 0)] + [(load_w1, 1, g) for g in (5, 0)] + [(load_obs, 3, 4)] + [(load_w1, 1, g) for g in (3, 1, 2)] + rows_of(3)[1:]
         sync_q += [(load_w2, piece) for piece in W2_PIECES[1::-1] + W2_PIECES[2:]] + [(load_b2,), (load_eps,)] + stores
 
-        tensor_q = [(turn, q, g) for q in GROUPS[0] for g in (4, 5)] + turns(front(0)) + turns(front(2)) + [(front_pass, 0, 4)]
+        tensor_q = [(turn, 0, 4), (turn, 0, 5), (warm_up, 0), (turn, 1, 4), (turn, 1, 5), (warm_up, 1)] + turns(front(0)) + [(warm_up, 2)] + turns(front(2)) + [(front_pass, 0, 4)]
         tensor_q += [(front_pass, 0, 5, 0, 2)] + turns(front(1)) + [(front_pass, 0, 5, 2, 4)] + turns(front(3))
-        tensor_q += [(front_pass, 0, 0)] + turns((2, 4)) + [(front_pass, 0, 2), (front_pass, 0, 1), (front_pass, 0, 3)] + turns((2, 0))
-        tensor_q += [(pass_w1, whole(1, 0), 0), (pass_w1, whole(1, 0), 1)] + turns((2, 2)) + [(front_pass, 1, 4), (front_pass, 1, 5)]
+        tensor_q += [(front_pass, 0, 0)] + turns((2, 4)) + [(front_pass, 0, 2), (front_pass, 0, 1)] + turns((2, 0)) + [(front_pass, 0, 3)]
+        tensor_q += turns((2, 2)) + [(pass_w1, whole(1, 0), 0), (pass_w1, whole(1, 0), 1)] + [(front_pass, 1, 4), (front_pass, 1, 5)]
         tensor_q += turns((3, 4)) + [(front_pass, 1, 0), (fill_bank, THIRD, 0, 0)]
         tensor_q += [(front_pass, 1, 2), (front_pass, 1, 3), (front_pass, 1, 1), (fill_bank, THIRD, 0, 2)] + turns((3, 2))
         tensor_q += [(fill_bank, THIRD, 1, 0)] + turns((3, 0)) + [(fill_bank, THIRD, 1, 2), (heads, 0), (heads, 1)]
 
-        gpsimd_q = [by("gpsimd", shared(*key), 0, POOL_RUNS) for key in ((0, 5), (0, 2), (0, 3), (1, 5), (1, 3))]
+        gpsimd_q = [by("gpsimd", shared(0, 5), 0, RUNS // 2)] + [by("gpsimd", shared(*key), 0, POOL_RUNS) for key in ((0, 2), (0, 3), (1, 5), (1, 3))]
         gpsimd_q += [(weave_w2, W2_PIECES[1], "gpsimd"), (weave_h, FRONT_B, 0, "gpsimd")]
 
-        scalar_q = [(widen, 0, 4, "scalar"), by("scalar", first, HEAD_RUNS)] + widens(1, 4) + [by("scalar", shared(0, 5), POOL_RUNS)] + widens(0, 2) + [(drain, 0, 0)] + widens(1, 2) + [(drain, 1, 0)]
-        scalar_q += [by("scalar", whole(0, 0)), by("scalar", shared(0, 2), POOL_RUNS)] + empties(front(1)) + [(widen_both, 2, 4)]
-        scalar_q += [by("scalar", whole(0, 1)), by("scalar", shared(0, 3), POOL_RUNS), by("scalar", whole(1, 4), LATE_RUNS)] + widens(2, 2) + [by("scalar", shared(1, 5), POOL_RUNS)]
-        scalar_q += [(relu, FRONT, 0, 0)] + empties((2, 0)) + [(relu, FRONT, 0, 2), (drain_w1, whole(1, 0), 0), (drain_w1, whole(1, 0), 1), (widen_both, 3, 4)]
+        scalar_q = [(widen, 0, 4, "scalar"), by("scalar", first, HEAD_RUNS)] + widens(1, 4) + [by("scalar", shared(0, 5), RUNS // 2)] + widens(0, 2) + [(drain, 0, 0)] + widens(1, 2) + [(drain, 1, 0)]
+        scalar_q += [by("scalar", whole(0, 0)), by("scalar", shared(0, 2), POOL_RUNS)] + [(widen_both, 2, 4)] + empties(front(1))
+        scalar_q += [by("scalar", whole(0, 1)), by("scalar", shared(0, 3), POOL_RUNS), by("scalar", whole(1, 4))] + widens(2, 2) + [by("scalar", shared(1, 5), POOL_RUNS)]
+        scalar_q += empties((2, 0)) + relus(FRONT, 0) + [ (drain_w1, whole(1, 0), 0), (drain_w1, whole(1, 0), 1), (widen_both, 3, 4)]
         scalar_q += [by("scalar", whole(1, 2)), by("scalar", shared(1, 3), POOL_RUNS)] + widens(3, 2) + [(weave_h, FRONT_A, 0, "scalar"), (relu, THIRD, 0, 0)]
         scalar_q += [(weave_w2, W2_PIECES[0], "scalar"), (weave_w2, W2_PIECES[3], "scalar")] + relus(FRONT, 1) + [(relu, THIRD, 0, 2)]
         scalar_q += [(weave_h, FRONT_A, 1, "scalar")] + empties((3, 0)) + [(weave_h, FRONT_B, 1, "scalar")] + relus(THIRD, 1)
@@ -417,7 +416,7 @@ def tile_rssm_pa_kernel(tc, prev_state, prev_action, obs_bytes, obs_scale, eps,
         vector_q += [(quant_x, front(4)), (quant_w1, shared(0, 5)), (quant_x, front(5))]
         vector_q += empties(front(2)) + [(quant_x, front(0)), (quant_w1, whole(0, 0)), (quant_x, front(2)), (quant_w1, shared(0, 2))]
         vector_q += empties(front(3)) + [(quant_x, front(1)), (quant_w1, whole(0, 1)), (quant_x, front(3)), (quant_w1, shared(0, 3))]
-        vector_q += empties((2, 4)) + [by("vector", whole(1, 4), 0, LATE_RUNS), (quant_x, (2, 4)), (quant_w1, whole(1, 4)), (quant_w1, shared(1, 5))]
+        vector_q += empties((2, 4)) + [(quant_w1, whole(1, 4)), (quant_x, (2, 4)), (quant_w1, shared(1, 5))]
         vector_q += empties((2, 2)) + [(quant_w1, whole(1, 0)), (quant_x, (2, 2)), (quant_x, (2, 0)), by("vector", whole(1, 1))]
         vector_q += [(quant_w1, whole(1, 2)), (quant_w1, shared(1, 3)), (quant_w1, whole(1, 1))]
         vector_q += empties((3, 4)) + [(weave_w2, W2_PIECES[2], "vector"), (quant_x, (3, 4))]

@@ -23,22 +23,68 @@ G2 = H // KP
 NT = B // P
 QT = 2 * P
 STATE_PASSES = S // KP
+MIXED, LATE = STATE_PASSES, STATE_PASSES + 2
 WOVEN = 4 * KP
-ACTION_ROWS = A // 4
-
-GROUPS = ((0, 1), (2,), (3,))
-FRONT, THIRD, LAST, LAST_A, LAST_B = (0, 0, 2 * QT), (1, 0, QT), (2, 0, QT), (2, 0, P), (2, P, P)
-SPLIT = 2 * L - KP
-ALL_PASSES, FIRST_PASS, SECOND_PASS = (0, 1), (0,), (1,)
-W2_PIECES = tuple((g, c0, min(KP, 2 * L - c0)) for g in range(G2) for c0 in (0, KP))
 RUNS = KP // 8
-ORDER = ((4, 5, 0, 2, 1, 3), (4, 5, 0, 2, 3, 1))
-DEPTH = {"wraw": 6, "woven_w": 3, "woven_g": 1, "woven_v": 1, "woven_s": 3, "woven_x": 3, "res": 4,
-         "state1": 4, "state2": 1, "wide2": 8, "wide4": 2, "obs2": 2, "obs4": 2}
-HIDDEN_DEPTH = {2 * QT: 2, QT: 3, P: 2}
-HEAD_RUNS = 34
-FRONT_A, FRONT_B = (0, 0, QT), (0, QT, QT)
-POOL_RUNS = 48
+ACTION_ROWS = A // 4
+SPLIT = 2 * L - KP
+
+GROUP_TOKENS = (2 * QT, QT, QT)
+FRONT, FRONT_A, FRONT_B = (0, 0, 2 * QT), (0, 0, QT), (0, QT, QT)
+THIRD, LAST, LAST_A, LAST_B = (1, 0, QT), (2, 0, QT), (2, 0, P), (2, P, P)
+W2_PIECES = tuple((g, c0, min(KP, 2 * L - c0)) for g in range(G2) for c0 in (0, KP))
+H_PIECES = ((FRONT_A, 0), (FRONT_B, 0), (FRONT_A, 1), (FRONT_B, 1), (THIRD, 0), (THIRD, 1), (LAST, 0), (LAST_A, 1), (LAST_B, 1))
+CUT = 2 * KP - A
+OBS_LOADS = ((0, 1, CUT, O), (1, 1, CUT, O), (2, 2, CUT, O), (0, 2, 0, CUT), (2, 2, 0, CUT), (4, 2, 0, O), (6, 2, 0, O))
+
+
+def rotate(keys, depth):
+    return [keys[i::depth] for i in range(depth)]
+
+
+def turned(*pairs):
+    return [("turn",) + pair for pair in pairs]
+
+
+def w(*pairs):
+    return [("w",) + pair for pair in pairs]
+
+
+W1_LOADS = [(0, 4), (0, 5), (0, 2), (0, 3), (0, 0), (0, 1), (1, 4), (1, 5), (1, 0), (1, 1), (1, 2), (1, 3)]
+HEADS = rotate([("head", n, c0) for n in range(NT) for c0 in (SPLIT, 0)], 4)
+BANKS = [
+    turned((0, 4), (0, 2), (0, 0), (2, 4), (2, 0)) + [("acc", THIRD, 0, 0)] + turned((3, 3)) + [("acc", THIRD, 1, 0), ("acc", LAST, 0, 2), ("acc", LAST_B, 1, 1)],
+    turned((0, 5), (0, 3), (0, 1), (2, 5), (2, 1), (3, 2), (3, 1)) + [("acc", LAST, 0, 0), ("acc", LAST_B, 1, 0)],
+    turned((1, 4), (1, 2), (1, 0), (2, 2), (3, 4)) + [("acc", THIRD, 0, 2), ("acc", THIRD, 1, 2), ("acc", LAST_B, 1, 2)],
+    turned((1, 5), (1, 3), (1, 1), (2, 3), (3, 5), (3, 0)) + [("acc", LAST_A, 1, 0), ("acc", LAST_B, 1, 3)],
+] + [[("acc", FRONT, 0, t), ("acc", FRONT, 1, t)] + HEADS[t] for t in range(4)]
+WOVEN_LISTS = [
+    w((0, 5), (0, 3), (1, 0)) + [("w2", 1, 0)],
+    w((0, 4), (0, 1), (1, 5), (1, 3)) + [("w2", 0, 0)],
+    w((0, 2), (1, 4), (1, 2)),
+    w((0, 0), (1, 1)) + [("w2", 1, KP)],
+]
+NARROW_LISTS = rotate([("h", FRONT_A, 0), ("h", FRONT_B, 0), ("w2", 0, KP), ("h", FRONT_A, 1), ("h", FRONT_B, 1),
+                       ("h", THIRD, 0), ("h", THIRD, 1), ("h", LAST, 0), ("h", LAST_A, 1), ("h", LAST_B, 1)], 4)
+SLICES_A_BANK = {FRONT: 1, THIRD: 2, LAST: 2, LAST_A: 4, LAST_B: 1}
+LAST_BIAS = ((L, L + L // 2), (L + L // 2, 2 * L), (0, SPLIT), (SPLIT, L))
+BUFFERS = {
+    "bank": ("psum", [P, KP], F32, BANKS),
+    "obs": ("keep", [P, 2 * O], U8, [[("obs", 0, CUT), ("obs", 4, 0)], [("obs", 1, CUT), ("obs", 6, 0)]]),
+    "obs_front": ("keep", [P, 4 * KP], U8, [[("obs", 2, CUT)], [("obs", 0, 0)], [("obs", 2, 0)]]),
+    "wide": ("keep", [P, 4 * KP], BF16, [[("wide", q, g), ("wide", q + 2, g)] for q in range(2) for g in (MIXED, LATE)]),
+    "state": ("keep", [P, 2, S], BF16, rotate([("state", q) for q in range(4)], 3)),
+    "raw": ("keep", [P, 4, KP], BF16, rotate([("raw",) + key for key in W1_LOADS], 6)),
+    "raw2": ("keep", [P, 4, 2 * L], BF16, rotate([("raw2", g) for g in range(G2)], 2)),
+    "woven": ("keep", [P, WOVEN], BF16, WOVEN_LISTS),
+    "narrow": ("keep", [P, WOVEN // 2], BF16, NARROW_LISTS),
+    "woven_x": ("keep", [P, WOVEN], BF16, rotate([("x", 0, g) for g in (4, 5, 2, 3, 0, 1)] + [("x", grp, g) for grp in (1, 2) for g in (4, 2, 0)], 4)),
+    "hidden": ("keep", [P, WOVEN], BF16, [[("hidden", FRONT, half)] for half in range(2)]),
+    "hidden_late": ("keep", [P, WOVEN // 2], BF16, rotate([("hidden", THIRD, 0), ("hidden", THIRD, 1), ("hidden", LAST, 0),
+                                                           ("hidden", LAST_A, 1)], 3)),
+    "res": ("keep", [P, 2 * L], F32, rotate([("res", n) for n in range(NT)], 4)),
+    "sample": ("keep", [P, L], F32, rotate([("sample", n) for n in range(NT)], 4)),
+}
 
 
 def tile_rssm_pa_kernel(tc, prev_state, prev_action, obs_bytes, obs_scale, eps,
@@ -55,8 +101,7 @@ def tile_rssm_pa_kernel(tc, prev_state, prev_action, obs_bytes, obs_scale, eps,
 
     with ExitStack() as ctx:
         keep = ctx.enter_context(tc.tile_pool(name="keep", bufs=1))
-        stream = ctx.enter_context(tc.tile_pool(name="stream", bufs=1))
-        psum = ctx.enter_context(tc.psum_pool(name="psum", bufs=4))
+        psum = ctx.enter_context(tc.psum_pool(name="psum", bufs=1))
         ctx.enter_context(tc.manual_schedule())
 
         w1c = keep.tile([P, G1, H], U32, align_bytes=64)
@@ -64,73 +109,68 @@ def tile_rssm_pa_kernel(tc, prev_state, prev_action, obs_bytes, obs_scale, eps,
         w2c = keep.tile([P, G2, 2 * L], U32, align_bytes=64)
         w2s = keep.tile([P, G2, 2 * L], U8, align_bytes=64)
         xc, xs, hc, hs = [], [], [], []
-        for grp, quarters in enumerate(GROUPS):
-            n = QT * len(quarters)
+        for grp, n in enumerate(GROUP_TOKENS):
             xc.append(keep.tile([P, G1, n], U32, name="xc%d" % grp, align_bytes=64))
             xs.append(keep.tile([P, G1, n], U8, name="xs%d" % grp, align_bytes=64))
             hc.append(keep.tile([P, G2, n], U32, name="hc%d" % grp, align_bytes=64))
             hs.append(keep.tile([P, G2, n], U8, name="hs%d" % grp, align_bytes=64))
         scale_mixed = keep.tile([P, 4], F32)
-        scale_obs = keep.tile([P, G1 - STATE_PASSES - 1, 4], F32)
+        scale_obs = keep.tile([P, G1 - MIXED - 1, 4], F32)
         ones = keep.tile([ACTION_ROWS, 4], F32)
         b1_cols = keep.tile([P, G2, 4], BF16)
         b2_rows = keep.tile([P, 2 * L], BF16)
         eps_sb = keep.tile([P, NT, L], BF16)
         ident = keep.tile([P, P], F32)
-        ident_bf = keep.tile([P, P], BF16)
 
-        raw, woven, rows, obs, banks, hidden, result = {}, {}, {}, {}, {}, {}, {}
+        tile_of, before = {}, {}
+        for family, (pool_name, shape, dtype, lists) in BUFFERS.items():
+            for i, keys in enumerate(lists):
+                if pool_name == "psum":
+                    buf = psum.tile(shape, dtype, name="%s%d" % (family, i))
+                else:
+                    buf = keep.tile(shape, dtype, name="%s%d" % (family, i), align_bytes=64)
+                for j, key in enumerate(keys):
+                    tile_of[key] = buf
+                    if j:
+                        before[key] = keys[j - 1]
+
         copy = {"vector": nc.vector.tensor_copy, "scalar": nc.scalar.copy}
 
-        def streamed(tag, shape, dtype):
-            return stream.tile(shape, dtype, name=tag, bufs=DEPTH[tag], align_bytes=64)
+        def gpsimd_copy(out, in_):
+            nc.gpsimd.tensor_scalar(out=out, in0=in_, scalar1=1.0, scalar2=0.0, op0=ALU.mult, op1=ALU.add)
 
         def load_scales():
-            first = KP - A
             flat = obs_scale.rearrange("o k -> (o k)")
-            nc.sync.dma_start(out=scale_obs[:], in_=flat[first:].rearrange("(g p t) -> p g t", p=P, t=4))
-            mixed = flat[:first].rearrange("(p t) -> p t", t=4)
+            nc.sync.dma_start(out=scale_obs[:], in_=flat[KP - A:].rearrange("(g p t) -> p g t", p=P, t=4))
+
+        def load_mixed_scales():
+            mixed = obs_scale.rearrange("o k -> (o k)")[:KP - A].rearrange("(p t) -> p t", t=4)
             for p0, p1 in ((ACTION_ROWS, P // 2), (P // 2, P)):
                 nc.sync.dma_start(out=scale_mixed[p0:p1, :], in_=mixed[p0 - ACTION_ROWS:p1 - ACTION_ROWS, :])
 
         def load_w1(half, g):
-            raw[half, g] = streamed("wraw", [P, 4, KP], BF16)
-            nc.sync.dma_start(out=raw[half, g][:], in_=w1_v[g][:, :, KP * half:KP * half + KP])
+            nc.sync.dma_start(out=tile_of["raw", half, g][:], in_=w1_v[g][:, :, KP * half:KP * half + KP])
 
-        def load_w2(piece):
-            g, c0, n = piece
-            raw[piece] = streamed("wraw", [P, 4, n], BF16)
-            nc.sync.dma_start(out=raw[piece][:], in_=w2_v[g][:, :, c0:c0 + n])
+        def load_w2(g):
+            nc.sync.dma_start(out=tile_of["raw2", g][:], in_=w2_v[g])
 
-        def load_state(q, g):
-            n = 1 if q in GROUPS[0] else STATE_PASSES
-            buf = streamed("state%d" % n, [P, 2, n * KP], BF16)
-            for i in range(2):
-                for j in range(n):
-                    rows[2 * q + i, g + j] = buf[:, i, KP * j:KP * j + KP]
-            nc.sync.dma_start(out=buf[:], in_=state_v[:, 2 * q:2 * q + 2, KP * g:KP * (g + n)])
+        def load_state(q):
+            nc.sync.dma_start(out=tile_of["state", q][:], in_=state_v[:, 2 * q:2 * q + 2, :])
 
         def obs_cols(g):
             return max(KP * g - S - A, 0), KP * (g + 2) - S - A
 
-        def load_obs(q, g):
+        def load_obs(n0, tiles, c0, c1):
+            nc.sync.dma_start(out=tile_of["obs", n0, c0][:, :tiles * (c1 - c0)].rearrange("p (i c) -> p i c", i=tiles),
+                              in_=bytes_v[:, n0:n0 + tiles, c0:c1])
+
+        def obs_load_of(n, g):
             c0, c1 = obs_cols(g)
-            obs[q, g] = streamed("obs%d" % g, [P, 2, c1 - c0], U8)
-            nc.sync.dma_start(out=obs[q, g][:], in_=bytes_v[:, 2 * q:2 * q + 2, c0:c1])
+            return [a for a in OBS_LOADS if a[0] <= n < a[0] + a[1] and a[2] <= c0 and c1 <= a[3]][0]
 
-        def wide_tile(n, g):
-            if (n, g) not in rows:
-                tiles = 1 if g == STATE_PASSES else 2
-                buf = streamed("wide%d" % g, [P, tiles * 2 * KP], BF16)
-                rows[n, g, "all"] = buf[:]
-                for i in range(tiles):
-                    part = buf[:, 2 * KP * i:2 * KP * (i + 1)]
-                    rows[n + i, g, "tile"] = part
-                    rows[n + i, g], rows[n + i, g + 1] = part[:, :KP], part[:, KP:]
-            return rows[n, g, "tile"]
-
-        def load_action(n):
-            nc.sync.dma_start(out=wide_tile(n, STATE_PASSES)[:, :A], in_=action_v[:, n, :])
+        def load_action(q):
+            out = tile_of["wide", q, MIXED][:].rearrange("p (i c) -> p i c", i=2)[:, :, :A]
+            nc.sync.dma_start(out=out, in_=action_v[:, 2 * q:2 * q + 2, :])
 
         def load_b1():
             nc.sync.dma_start(out=b1_cols[:], in_=b1.rearrange("(g p t) -> p g t", p=P, t=4))
@@ -143,432 +183,311 @@ def tile_rssm_pa_kernel(tc, prev_state, prev_action, obs_bytes, obs_scale, eps,
 
         def widen(n, g, engine):
             c0, c1 = obs_cols(g)
-            copy[engine](out=wide_tile(n, g)[:, 2 * KP - (c1 - c0):], in_=obs[n // 2, g][:, n % 2, :].bitcast(FP8))
+            n0, tiles, l0, l1 = obs_load_of(n, g)
+            at = (n - n0) * (l1 - l0) + c0 - l0
+            end = 2 * KP * (n % 2 + 1)
+            copy[engine](out=tile_of["wide", n // 2, g][:, end - (c1 - c0):end],
+                         in_=tile_of["obs", n0, l0][:, at:at + c1 - c0].bitcast(FP8))
 
-        def widen_both(q, g):
-            wide_tile(2 * q, g)
-            nc.scalar.copy(out=rows[2 * q, g, "all"], in_=obs[q, g][:].rearrange("p i c -> p (i c)").bitcast(FP8))
+        def rows(n, g):
+            if g < STATE_PASSES:
+                return tile_of["state", n // 2][:, n % 2, KP * g:KP * g + KP]
+            at = 2 * KP * (n % 2) + KP * (g % 2)
+            return tile_of["wide", n // 2, g - g % 2][:, at:at + KP]
 
         def turn(q, g):
-            banks[q, g] = psum.tile([P, 2, QT], F32, name=turn_tag(q, g))
+            bank = tile_of["turn", q, g][:].rearrange("p (u r) -> p u r", u=2)
             for i in range(2):
-                words = rows[2 * q + i, g].bitcast(F32)
+                words = rows(2 * q + i, g).bitcast(F32)
                 for u in range(2):
-                    nc.tensor.transpose(banks[q, g][:, u, P * i:P * i + P], words[:, u::2], ident[:])
+                    nc.tensor.transpose(bank[:, u, P * i:P * i + P], words[:, u::2], ident[:])
 
-        def pair_of(q, g):
-            return (("front", g), q) if q in GROUPS[0] else ((q, g - g % 2), g % 2)
-
-        def banks_of(pair):
-            return [(q, pair[1]) for q in GROUPS[0]] if pair[0] == "front" else [pair, (pair[0], pair[1] + 1)]
+        def x_key(q, g):
+            return (("x", 0, g), q) if q < 2 else (("x", q - 1, g - g % 2), g % 2)
 
         def x_half(q, g):
-            pair, j = pair_of(q, g)
-            if ("x", pair) not in woven:
-                woven["x", pair] = streamed("woven_x", [P, WOVEN], BF16)
-            return woven["x", pair][:, WOVEN // 2 * j:WOVEN // 2 * (j + 1)]
+            key, j = x_key(q, g)
+            return tile_of[key][:, WOVEN // 2 * j:WOVEN // 2 * (j + 1)]
 
         def drain(q, g):
-            out = x_half(q, g).bitcast(F32).rearrange("p (r u) -> p r u", u=2)
-            nc.scalar.copy(out=out, in_=banks[q, g][:].rearrange("p u r -> p r u"))
+            nc.scalar.copy(out=x_half(q, g).bitcast(F32).rearrange("p (r u) -> p r u", u=2),
+                           in_=tile_of["turn", q, g][:].rearrange("p (u r) -> p r u", u=2))
 
         def product(q, g):
-            scale = scale_mixed[:] if g == STATE_PASSES else scale_obs[:, g - STATE_PASSES - 1, :]
+            scale = scale_mixed[:] if g == MIXED else scale_obs[:, g - MIXED - 1, :]
             nc.vector.tensor_tensor(out=x_half(q, g).rearrange("p (r u e) -> p r u e", u=2, e=2),
-                                    in0=banks[q, g][:].bitcast(BF16).rearrange("p u (r e) -> p r u e", e=2),
+                                    in0=tile_of["turn", q, g][:].bitcast(BF16).rearrange("p (u r e) -> p r u e", u=2, e=2),
                                     in1=scale.rearrange("p (u e) -> p u e", e=2).unsqueeze(1).to_broadcast([P, QT, 2, 2]),
                                     op=ALU.mult)
 
-        def quant_x(pair):
-            grp, g0, n = (0, pair[1], 1) if pair[0] == "front" else (pair[0] - 1, pair[1], 2)
-            nc.vector.quantize_mx(out=xc[grp][:, g0:g0 + n, :].rearrange("p g n -> p (g n)").bitcast(FP8X4),
-                                  scales=xs[grp][:, g0:g0 + n, :].rearrange("p g n -> p (g n)"), in_=woven["x", pair][:])
+        def quant_x(grp, g):
+            n = 1 if grp == 0 else 2
+            nc.vector.quantize_mx(out=xc[grp][:, g:g + n, :].rearrange("p g n -> p (g n)").bitcast(FP8X4),
+                                  scales=xs[grp][:, g:g + n, :].rearrange("p g n -> p (g n)"), in_=tile_of["x", grp, g][:])
 
-        def quant_first(q):
-            g, cols = ORDER[0][0], slice(QT * q, QT * q + QT)
-            nc.vector.quantize_mx(out=xc[0][:, g, cols].bitcast(FP8X4), scales=xs[0][:, g, cols], in_=x_half(q, g))
-
-        def weave_w1(part, engine, r0, r1):
-            half, g, s0, s1, tag = part
-            if part not in woven:
-                woven[part] = streamed(tag, [P, KP * (s1 - s0)], BF16)
+        def weave_w1(half, g, engine, r0, r1):
+            woven, raw = tile_of["w", half, g][:], tile_of["raw", half, g][:]
             if engine == "gpsimd":
-                nc.gpsimd.tensor_scalar(out=woven[part][:].rearrange("p (s m t) -> p m s t", m=P, t=4)[:, 2 * r0:2 * r1],
-                                        in0=raw[half, g][:].rearrange("p t (m s) -> p m s t", s=4)[:, 2 * r0:2 * r1, s0:s1],
-                                        scalar1=1.0, scalar2=0.0, op0=ALU.mult, op1=ALU.add)
+                gpsimd_copy(woven.rearrange("p (s m t) -> p m s t", m=P, t=4)[:, 2 * r0:2 * r1],
+                            raw.rearrange("p t (m s) -> p m s t", s=4)[:, 2 * r0:2 * r1])
             else:
-                copy[engine](out=woven[part][:].rearrange("p (s r e t) -> p r t e s", r=RUNS, e=2, t=4)[:, r0:r1],
-                             in_=raw[half, g][:].rearrange("p t (r e s) -> p r t e s", e=2, s=4)[:, r0:r1, :, :, s0:s1])
+                copy[engine](out=woven.rearrange("p (s r e t) -> p r t e s", r=RUNS, e=2, t=4)[:, r0:r1],
+                             in_=raw.rearrange("p t (r e s) -> p r t e s", e=2, s=4)[:, r0:r1])
 
-        def pass_w1(part, k):
-            half, g = part[:2]
-            banks[part, k] = psum.tile([P, 2 * P, 2, 2], BF16, name="tp")
-            cols = raw[half, g][:, :, 2 * P * k:2 * P * (k + 1)]
-            for u in range(2):
-                nc.tensor.matmul(banks[part, k][:, :, u, :], ident_bf[:], cols[:, 2 * u:2 * u + 2, :].rearrange("p e c -> p c e"),
-                                 start=True, stop=True)
+        def quant_w1(half, g):
+            cols = slice(KP * half, KP * half + KP)
+            nc.vector.quantize_mx(out=w1c[:, g, cols].bitcast(FP8X4), scales=w1s[:, g, cols], in_=tile_of["w", half, g][:])
 
-        def drain_w1(part, k):
-            if k == 0:
-                woven[part] = streamed(part[4], [P, WOVEN], BF16)
-            m0 = 2 * P * k // 4
-            out = woven[part][:].bitcast(F32).rearrange("p (s m w) -> p m s w", s=4, w=2)[:, m0:m0 + 2 * P // 4]
-            src = banks[part, k][:].rearrange("p c u e -> p (c u e)").bitcast(F32)
-            nc.scalar.copy(out=out, in_=src.rearrange("p (m s w) -> p m s w", s=4, w=2))
-
-        def quant_w1(part):
-            half, g, s0, s1, tag = part
-            cols = slice(KP * half + P * s0, KP * half + P * s1)
-            nc.vector.quantize_mx(out=w1c[:, g, cols].bitcast(FP8X4), scales=w1s[:, g, cols], in_=woven[part][:])
-
-        def weave_tag(engine):
-            return {"vector": "woven_v", "scalar": "woven_s", "gpsimd": "woven_g"}[engine]
-
-        def weave(key, src, engine):
-            woven[key] = streamed(weave_tag(engine), [P, 4 * src.shape[2]], BF16)[:]
+        def weave(woven, src, engine):
             if engine == "gpsimd":
-                nc.gpsimd.tensor_scalar(out=woven[key].rearrange("p (c t) -> p c t", t=4), in0=src.rearrange("p t c -> p c t"),
-                                        scalar1=1.0, scalar2=0.0, op0=ALU.mult, op1=ALU.add)
+                gpsimd_copy(woven.rearrange("p (c t) -> p c t", t=4), src.rearrange("p t c -> p c t"))
             else:
-                copy[engine](out=woven[key].rearrange("p (r e t) -> p r t e", e=8, t=4),
+                copy[engine](out=woven.rearrange("p (r e t) -> p r t e", e=8, t=4),
                              in_=src.rearrange("p t (r e) -> p r t e", e=8))
 
-        def weave_w2(piece, engine):
-            weave(piece, raw[piece][:], engine)
+        def weave_w2(g, c0, n, engine, r0, r1):
+            weave(tile_of["w2", g, c0][:, 32 * r0:32 * r1], tile_of["raw2", g][:, :, c0 + 8 * r0:c0 + 8 * r1], engine)
 
-        def quant_w2(piece):
-            g, c0, n = piece
-            nc.vector.quantize_mx(out=w2c[:, g, c0:c0 + n].bitcast(FP8X4), scales=w2s[:, g, c0:c0 + n], in_=woven[piece])
+        def quant_w2(g, c0, n):
+            nc.vector.quantize_mx(out=w2c[:, g, c0:c0 + n].bitcast(FP8X4), scales=w2s[:, g, c0:c0 + n],
+                                  in_=tile_of["w2", g, c0][:, :4 * n])
 
-        def mm1(span, half, t, g):
+        def sums(span, half, t):
+            n = span[2]
+            first = t - t % SLICES_A_BANK[span]
+            return ("acc", span, half, first), n * (t - first)
+
+        def pairs_of(slices, passes):
+            return [(t, g) for t in slices for g in passes] if len(passes) == G1 else [(t, g) for g in passes for t in slices]
+
+        def mm1(span, half, slices, passes):
             grp, r0, n = span
-            sums = banks[FRONT, half, t][:, r0:r0 + n] if grp == 0 else banks[span, half, t]
-            cols = slice(KP * half + P * t, KP * half + P * t + P)
-            nc.tensor.matmul_mx(out=sums, lhsT=w1c[:, g, cols].bitcast(FP8X4), lhsT_scale=w1s[:, g, cols],
-                                rhs=xc[grp][:, g, r0:r0 + n].bitcast(FP8X4), rhs_scale=xs[grp][:, g, r0:r0 + n],
-                                start=(g == ORDER[half][0] and (grp > 0 or r0 == 0)), stop=(g == ORDER[half][-1]))
+            for t, g in pairs_of(slices, passes):
+                key, at = sums(span, half, t)
+                cols = slice(KP * half + P * t, KP * half + P * t + P)
+                nc.tensor.matmul_mx(out=tile_of[key][:, at:at + n], lhsT=w1c[:, g, cols].bitcast(FP8X4), lhsT_scale=w1s[:, g, cols],
+                                    rhs=xc[grp][:, g, r0:r0 + n].bitcast(FP8X4), rhs_scale=xs[grp][:, g, r0:r0 + n],
+                                    start=(in_bank[key][0] == (t, g)), stop=(in_bank[key][-1] == (t, g)))
 
-        def front_pass(half, g, t0=0, t1=4):
-            for t in range(t0, t1):
-                if g == ORDER[half][0]:
-                    acc = psum.tile([P, KP], F32, name="acc")
-                    banks[FRONT, half, t] = acc[:]
-                mm1(FRONT, half, t, g)
-
-        def first_pass(q):
-            for t in range(4):
-                if q == 0:
-                    acc = psum.tile([P, KP], F32, name="acc")
-                    banks[FRONT, 0, t] = acc[:]
-                mm1((0, QT * q, QT), 0, t, ORDER[0][0])
-
-        def warm_up(k):
-            idle = psum.tile([P, KP], F32, name="acc")
-            for j in range(2):
-                nc.tensor.matmul(idle[:], ident_bf[:], rows[0, ORDER[0][0]], start=True, stop=True)
-
-        def bank_start(span, t):
-            return t - t % (KP // span[2])
-
-        def fill_bank(span, half, t0):
+        def relu(span, half, t):
+            key, at = sums(span, half, t)
             n = span[2]
-            acc = psum.tile([P, KP // n, n], F32, name=bank_tag(span, half))
-            for t in range(t0, t0 + KP // n):
-                banks[span, half, t] = acc[:, t - t0, :]
-                for g in ORDER[half]:
-                    mm1(span, half, t, g)
+            nc.scalar.activation(tile_of["hidden", span, half][:, n * t:n * t + n], tile_of[key][:, at:at + n], ACT.Relu,
+                                 bias=b1_cols[:, half, t:t + 1])
 
-        def relu(span, half, t0):
+        def relu_woven(span, half, t):
+            key, at = sums(span, half, t)
             n = span[2]
-            if t0 == 0:
-                hidden[span, half] = stream.tile([P, 4, n], BF16, name="hidden%d" % n, bufs=HIDDEN_DEPTH[n])
-            for t in (t0, t0 + 1):
-                nc.scalar.activation(hidden[span, half][:, t, :], banks[span, half, t], ACT.Relu,
-                                     bias=b1_cols[:, half, t:t + 1])
+            out = tile_of["h", span, half][:, :4 * n].rearrange("p (n t) -> p n t", t=4)[:, :, t]
+            nc.scalar.activation(out, tile_of[key][:, at:at + n], ACT.Relu, bias=b1_cols[:, half, t:t + 1])
+
+        def parent(span):
+            return FRONT if span[0] == 0 else span
 
         def weave_h(span, half, engine):
-            grp, r0, n = span
-            src = hidden[FRONT, half][:, :, r0:r0 + n] if grp == 0 else hidden[span, half][:]
-            weave((span, half), src, engine)
+            whole = parent(span)
+            src = tile_of["hidden", whole, half][:, :4 * whole[2]].rearrange("p (t n) -> p t n", t=4)
+            r0 = span[1] - whole[1]
+            weave(tile_of["h", span, half][:, :4 * span[2]], src[:, :, r0:r0 + span[2]], engine)
 
         def quant_h(span, half):
             grp, r0, n = span
             nc.vector.quantize_mx(out=hc[grp][:, half, r0:r0 + n].bitcast(FP8X4), scales=hs[grp][:, half, r0:r0 + n],
-                                  in_=woven[span, half])
+                                  in_=tile_of["h", span, half][:, :4 * n])
 
-        def spans_of(n):
-            piece = FRONT if (FRONT, 0) in weaver else (0, QT * (n // 2), QT)
-            front, third = [(piece, 0), (piece, 1)], [(THIRD, 0), (THIRD, 1)]
-            return front if n < 4 else third if n < 6 else [(LAST, 0), ((LAST_A, LAST_B)[n - 6], 1)]
-
-        def heads(n, passes=ALL_PASSES):
+        def place(n):
             grp = max(n // 2 - 1, 0)
-            r0 = P * (n - 2 * GROUPS[grp][0])
+            return grp, P * (n - (0, 4, 6)[grp])
+
+        def heads(n, passes):
+            grp, r0 = place(n)
             for c0, c1 in ((SPLIT, 2 * L), (0, SPLIT)):
-                if 0 in passes:
-                    banks["head", n, c0] = psum.tile([P, c1 - c0], F32, name="tp")
                 for g in passes:
-                    nc.tensor.matmul_mx(out=banks["head", n, c0][:], lhsT=hc[grp][:, g, r0:r0 + P].bitcast(FP8X4),
+                    nc.tensor.matmul_mx(out=tile_of["head", n, c0][:, :c1 - c0], lhsT=hc[grp][:, g, r0:r0 + P].bitcast(FP8X4),
                                         lhsT_scale=hs[grp][:, g, r0:r0 + P], rhs=w2c[:, g, c0:c1].bitcast(FP8X4),
                                         rhs_scale=w2s[:, g, c0:c1], start=(g == 0), stop=(g == G2 - 1))
 
-        def bias_wide(n):
-            result[n] = streamed("res", [P, 2 * L], F32)
-            result[n, "sample"] = stream.tile([P, L], F32, name="sample", bufs=DEPTH["res"])
-            nc.vector.tensor_add(out=result[n][:, SPLIT:], in0=banks["head", n, SPLIT][:], in1=b2_rows[:, SPLIT:])
+        def bias_parts(n):
+            return LAST_BIAS if n == NT - 1 else ((SPLIT, 2 * L), (0, SPLIT))
 
-        def bias_narrow(n):
-            nc.vector.tensor_add(out=result[n][:, :SPLIT], in0=banks["head", n, 0][:], in1=b2_rows[:, :SPLIT])
+        def bias(n, c0, c1):
+            b0 = SPLIT if c0 >= SPLIT else 0
+            nc.vector.tensor_add(out=tile_of["res", n][:, c0:c1], in0=tile_of["head", n, b0][:, c0 - b0:c1 - b0], in1=b2_rows[:, c0:c1])
 
-        def root(n):
-            nc.scalar.activation(result[n, "sample"][:], result[n][:, L:], ACT.Sqrt)
+        def root(n, c0, c1):
+            nc.scalar.activation(tile_of["sample", n][:, c0:c1], tile_of["res", n][:, L + c0:L + c1], ACT.Sqrt)
 
-        def noise(n, c0=0, c1=L):
-            part = result[n, "sample"][:, c0:c1]
+        def noise(n, c0, c1):
+            part = tile_of["sample", n][:, c0:c1]
             nc.vector.tensor_mul(out=part, in0=part, in1=eps_sb[:, n, c0:c1])
 
-        def shift(n, c0=0, c1=L):
-            part = result[n, "sample"][:, c0:c1]
-            nc.vector.tensor_add(out=part, in0=part, in1=result[n][:, c0:c1])
+        def shift(n, c0, c1):
+            part = tile_of["sample", n][:, c0:c1]
+            nc.vector.tensor_add(out=part, in0=part, in1=tile_of["res", n][:, c0:c1])
 
-        def store_std(n):
-            nc.sync.dma_start(out=std_v[:, n, :], in_=result[n][:, L:])
+        def store_std(n, c0, c1):
+            nc.sync.dma_start(out=std_v[:, n, c0:c1], in_=tile_of["res", n][:, L + c0:L + c1])
 
         def store_mean(n):
-            nc.sync.dma_start(out=mean_v[:, n, :], in_=result[n][:, :L])
+            nc.sync.dma_start(out=mean_v[:, n, :], in_=tile_of["res", n][:, :L])
 
-        def store_sample(n, c0=0, c1=L):
-            nc.sync.dma_start(out=sample_v[:, n, c0:c1], in_=result[n, "sample"][:, c0:c1])
+        def store_sample(n, c0, c1):
+            nc.sync.dma_start(out=sample_v[:, n, c0:c1], in_=tile_of["sample", n][:, c0:c1])
 
-        def turn_tag(q, g):
-            return "tp"
+        def touches(f, *a):
+            if f == load_obs:
+                return [], [("obs", a[0], a[2])]
+            if f == widen:
+                load = obs_load_of(*a[:2])
+                return [("obs", load[0], load[2])], [("wide", a[0] // 2, a[1])]
+            if f == turn:
+                q, g = a
+                return [("state", q) if g < STATE_PASSES else ("wide", q, g - g % 2)], [("turn", q, g)]
+            if f in (drain, product):
+                scales = [] if f == drain else ["mixed"] if a[1] == MIXED else ["scales"]
+                return [("turn",) + a] + scales, [x_key(*a)[0]]
+            if f == mm1:
+                span, half, slices, passes = a
+                x = [("xq", span[0], g if span[0] == 0 else g - g % 2) for g in passes]
+                return x + [("wq", half, g) for g in passes], [sums(span, half, t)[0] for t in slices]
+            if f == relu:
+                return [sums(*a)[0], "b1"], [("hidden",) + a[:2]]
+            if f == relu_woven:
+                return [sums(*a)[0], "b1"], [("h",) + a[:2]]
+            if f == bias:
+                n, c0, c1 = a
+                return [("head", n, SPLIT if c0 >= SPLIT else 0), "b2"], [("res", n), ("biased", n, c0)]
+            if f in (root, store_std):
+                n, c0, c1 = a
+                std = [("biased", n, b0) for b0, b1 in bias_parts(n) if b0 < L + c1 and L + c0 < b1]
+                return std, [("sample", n), ("root",) + a] if f == root else []
+            if f == noise:
+                n, c0, c1 = a
+                return [("root",) + a, "eps"], [("noise",) + a]
+            if f == weave_h:
+                return [("hidden", parent(a[0]), a[1])], [("h",) + a[:2]]
+            if f == heads:
+                grp, r0 = place(a[0])
+                h = [("hq", span, half) for span, half in H_PIECES
+                     if span[0] == grp and span[1] <= r0 < span[1] + span[2] and half in a[1]]
+                return h + [("w2q",) + piece[:2] for piece in W2_PIECES], [("head", a[0], SPLIT), ("head", a[0], 0)]
+            return {load_scales: ([], ["scales"]), load_mixed_scales: ([], ["mixed"]), load_b1: ([], ["b1"]),
+                    load_b2: ([], ["b2"]), load_eps: ([], ["eps"]),
+                    load_w1: ([], [("raw",) + a]), load_w2: ([], [("raw2",) + a]), load_state: ([], [("state",) + a]),
+                    load_action: ([], [("wide",) + a + (MIXED,)]),
+                    quant_x: ([("x",) + a], [("xq",) + a]),
+                    weave_w1: ([("raw",) + a[:2]], [("w",) + a[:2]]), quant_w1: ([("w",) + a], [("wq",) + a]),
+                    weave_w2: ([("raw2",) + a[:1]], [("w2",) + a[:2]]), quant_w2: ([("w2",) + a[:2]], [("w2q",) + a[:2]]),
+                    quant_h: ([("h",) + a], [("hq",) + a]),
+                    shift: ([("noise",) + a, ("res",) + a[:1]], [("shifted",) + a]),
+                    store_mean: ([("res",) + a], []),
+                    store_sample: ([("shifted",) + a, ("sample",) + a[:1]], [])}[f]
 
-        def bank_tag(span, half):
-            return "tp" if (span, half) == (THIRD, 0) else "acc"
+        SL = (0, 1, 2, 3)
 
-        def turns(pair):
-            return [(turn, q, g) for q, g in banks_of(pair)]
+        def by(engine, half, g, r0=0, r1=RUNS):
+            return (weave_w1, half, g, engine, r0, r1)
 
-        def empties(pair):
-            return [(drain if g < STATE_PASSES else product, q, g) for q, g in banks_of(pair)]
-
-        def relus(span, half):
-            return [(relu, span, half, 0), (relu, span, half, 2)]
-
-        def front(g):
-            return ("front", g)
-
-        def whole(half, g):
-            return (half, g, 0, 4, "woven_w")
-
-        def low(half, g):
-            return (half, g, 0, 2, "woven_g")
-
-        def high(half, g):
-            return (half, g, 2, 4, "woven_w")
-
-        def by(engine, part, r0=0, r1=RUNS):
-            return (weave_w1, part, engine, r0, r1)
-
-        def rows_of(q):
-            return [(load_obs, q, 4), (load_state, q, 0), (load_obs, q, 2), (load_action, 2 * q), (load_action, 2 * q + 1)]
+        def steps(f, *args):
+            return [(f,) + a for a in args]
 
         def widens(q, g):
             return [(widen, 2 * q, g, "scalar"), (widen, 2 * q + 1, g, "scalar")]
 
+        def relus(span, half, slices=SL):
+            return [(relu, span, half, t) for t in slices]
+
+        def wide(n):
+            return (bias, n, SPLIT, 2 * L)
+
+        def narrow(n):
+            return (bias, n, 0, SPLIT)
+
         halves = [(NT - 1, 0, L // 2), (NT - 1, L // 2, L)]
         stores = []
         for n in range(NT):
-            before = [(store_sample, n - 1)] if n else []
-            stores += [(store_std, n)] + (before + [(store_mean, n)] if n >= NT - 2 else [(store_mean, n)] + before)
+            earlier = [(store_sample, n - 1, 0, L)] if n else []
+            stores += [(store_std, n, 0, L)] + (earlier + [(store_mean, n)] if n >= NT - 2 else [(store_mean, n)] + earlier)
         stores += [(store_sample,) + part for part in halves]
 
-        def shared(half, g):
-            return (half, g, 0, 4, "woven_g")
+        obs = [(load_obs,) + a for a in OBS_LOADS]
+        w1_loads = [(load_w1,) + key for key in W1_LOADS]
+        sync_q = obs[:2] + [(load_scales,), obs[2]] + w1_loads[:2] + [obs[3], (load_action, 0), w1_loads[2], obs[4], (load_action, 1), (load_mixed_scales,)]
+        sync_q += w1_loads[3:6] + [(load_state, 0), (load_state, 1), obs[5], (load_action, 2), (load_b1,)]
+        sync_q += [w1_loads[6], w1_loads[7], obs[6], (load_action, 3), w1_loads[8], (load_state, 2)] + w1_loads[9:] + [(load_w2, 0), (load_w2, 1), (load_state, 3), (load_b2,), (load_eps,)] + stores
 
-        first, second = (0, 4, 0, 4, "woven_g"), (1, 5, 0, 4, "woven_g")
-        sync_q = [(load_obs, 0, 4), (load_w1, 0, 4), (load_scales,), (load_obs, 1, 4), (load_w1, 0, 5), (load_obs, 0, 2), (load_state, 0, 0), (load_state, 1, 0)]
-        sync_q += [(load_obs, 1, 2)] + [(load_action, n) for n in range(4)]
-        sync_q += [(load_w1, 0, 0), (load_w1, 0, 2), (load_state, 0, 1), (load_state, 1, 1), (load_obs, 2, 4), (load_w1, 0, 1), (load_w1, 0, 3), (load_b1,)]
-        sync_q += [(load_w1, 1, 4)] + rows_of(2)[2:] + [(load_state, 2, 0)] + [(load_w1, 1, g) for g in (5, 0)] + [(load_obs, 3, 4)] + [(load_w1, 1, g) for g in (3, 1, 2)] + rows_of(3)[1:]
-        sync_q += [(load_w2, piece) for piece in W2_PIECES[1::-1] + W2_PIECES[2:]] + [(load_b2,), (load_eps,)] + stores
+        ALL = (4, 5, 2, 3, 0, 1)
+        tensor_q = steps(turn, (0, 4), (0, 5), (1, 4), (1, 5), (0, 2), (0, 3)) + [(mm1, FRONT, 0, SL, (4,))] + steps(turn, (1, 2), (1, 3)) + [(mm1, FRONT, 0, SL, (5,))]
+        tensor_q += steps(turn, (0, 0), (0, 1), (1, 0), (1, 1)) + [(mm1, FRONT, 0, SL, (2, 3))]
+        tensor_q += steps(turn, (2, 4), (2, 5)) + [(mm1, FRONT, 0, SL, (0,))] + steps(turn, (2, 2), (2, 3)) + [(mm1, FRONT, 0, SL, (1,))]
+        tensor_q += steps(turn, (2, 0), (2, 1)) + [(mm1, FRONT, 1, SL, (4, 5)), (mm1, THIRD, 0, (0, 1), ALL[:4]), (mm1, THIRD, 0, (0, 1), ALL[4:])] + steps(turn, (3, 4), (3, 5)) + [(mm1, FRONT, 1, SL, (0, 2, 3))]
+        tensor_q += steps(turn, (3, 2), (3, 3)) + [(mm1, FRONT, 1, SL, (1,)), (mm1, THIRD, 0, (2, 3), ALL)] + steps(turn, (3, 0), (3, 1))
+        tensor_q += [(mm1, THIRD, 1, SL, ALL), (heads, 0, (0, 1)), (heads, 1, (0, 1)), (mm1, LAST, 0, (0, 1), ALL), (heads, 2, (0, 1))]
+        tensor_q += [(mm1, LAST, 0, (2, 3), ALL), (heads, 3, (0, 1)), (heads, 4, (0, 1)), (mm1, LAST_A, 1, SL, ALL), (heads, 5, (0, 1))]
+        tensor_q += [(mm1, LAST_B, 1, SL, ALL), (heads, 6, (0, 1)), (heads, 7, (0,)), (heads, 7, (1,))]
 
-        tensor_q = [(turn, 0, 4), (turn, 0, 5), (warm_up, 0), (turn, 1, 4), (turn, 1, 5), (warm_up, 1)] + turns(front(0)) + [(warm_up, 2)] + turns(front(2)) + [(front_pass, 0, 4)]
-        tensor_q += [(front_pass, 0, 5, 0, 2)] + turns(front(1)) + [(front_pass, 0, 5, 2, 4)] + turns(front(3))
-        tensor_q += [(front_pass, 0, 0)] + turns((2, 4)) + [(front_pass, 0, 2), (front_pass, 0, 1)] + turns((2, 0)) + [(front_pass, 0, 3)]
-        tensor_q += turns((2, 2)) + [(pass_w1, whole(1, 0), 0), (pass_w1, whole(1, 0), 1)] + [(front_pass, 1, 4), (front_pass, 1, 5)]
-        tensor_q += turns((3, 4)) + [(front_pass, 1, 0), (fill_bank, THIRD, 0, 0)]
-        tensor_q += [(front_pass, 1, 2), (front_pass, 1, 3), (front_pass, 1, 1), (fill_bank, THIRD, 0, 2)] + turns((3, 2))
-        tensor_q += [(fill_bank, THIRD, 1, 0)] + turns((3, 0)) + [(fill_bank, THIRD, 1, 2), (heads, 0), (heads, 1)]
+        gpsimd_q = [by("gpsimd", 0, 4, 0, 36), by("gpsimd", 0, 5, 0, 44), by("gpsimd", 0, 3, 0, 30), by("gpsimd", 0, 2, 24), by("gpsimd", 0, 0, 40)]
+        gpsimd_q += [by("gpsimd", 1, 5), by("gpsimd", 1, 0, 0, 20), (weave_w2, 0, 0, KP, "gpsimd", 0, 64), (weave_w2, 0, KP, SPLIT, "gpsimd", 0, 32)]
 
-        gpsimd_q = [by("gpsimd", shared(0, 5), 0, RUNS // 2)] + [by("gpsimd", shared(*key), 0, POOL_RUNS) for key in ((0, 2), (0, 3), (1, 5), (1, 3))]
-        gpsimd_q += [(weave_w2, W2_PIECES[1], "gpsimd"), (weave_h, FRONT_B, 0, "gpsimd")]
+        scalar_q = [(widen, 1, LATE, "scalar"), (widen, 3, LATE, "scalar"), by("scalar", 0, 4, 36), by("scalar", 0, 5, 44)]
+        scalar_q += widens(0, MIXED) + [by("scalar", 0, 2, 0, 24)] + widens(1, MIXED) + [by("scalar", 0, 3, 30), by("scalar", 0, 0, 0, 40), by("scalar", 0, 1)] + steps(drain, (0, 0), (0, 1), (1, 0), (1, 1))
+        scalar_q += widens(2, LATE) + widens(2, MIXED) + [by("scalar", 1, 4)] + relus(FRONT, 0) + steps(drain, (2, 0), (2, 1))
+        scalar_q += widens(3, LATE) + [by("scalar", 1, 2), by("scalar", 1, 3, 32)] + relus(THIRD, 0, (0, 1)) + widens(3, MIXED) + [(weave_w2, 1, 0, KP, "scalar", 0, 64)]
+        scalar_q += relus(FRONT, 1) + [(weave_h, FRONT_A, 0, "scalar")] + relus(THIRD, 0, (2, 3)) + steps(drain, (3, 0), (3, 1)) + [(weave_h, FRONT_B, 0, "scalar"), (weave_h, FRONT_B, 1, "scalar")] + relus(THIRD, 1)
 
-        scalar_q = [(widen, 0, 4, "scalar"), by("scalar", first, HEAD_RUNS)] + widens(1, 4) + [by("scalar", shared(0, 5), RUNS // 2)] + widens(0, 2) + [(drain, 0, 0)] + widens(1, 2) + [(drain, 1, 0)]
-        scalar_q += [by("scalar", whole(0, 0)), by("scalar", shared(0, 2), POOL_RUNS)] + [(widen_both, 2, 4)] + empties(front(1))
-        scalar_q += [by("scalar", whole(0, 1)), by("scalar", shared(0, 3), POOL_RUNS), by("scalar", whole(1, 4))] + widens(2, 2) + [by("scalar", shared(1, 5), POOL_RUNS)]
-        scalar_q += empties((2, 0)) + relus(FRONT, 0) + [ (drain_w1, whole(1, 0), 0), (drain_w1, whole(1, 0), 1), (widen_both, 3, 4)]
-        scalar_q += [by("scalar", whole(1, 2)), by("scalar", shared(1, 3), POOL_RUNS)] + widens(3, 2) + [(weave_h, FRONT_A, 0, "scalar"), (relu, THIRD, 0, 0)]
-        scalar_q += [(weave_w2, W2_PIECES[0], "scalar"), (weave_w2, W2_PIECES[3], "scalar")] + relus(FRONT, 1) + [(relu, THIRD, 0, 2)]
-        scalar_q += [(weave_h, FRONT_A, 1, "scalar")] + empties((3, 0)) + [(weave_h, FRONT_B, 1, "scalar")] + relus(THIRD, 1)
+        vector_q = [(widen, 0, LATE, "vector"), (widen, 2, LATE, "vector")] + steps(product, (0, 4), (0, 5), (1, 4), (1, 5))
+        vector_q += [(quant_w1, 0, 4), (quant_x, 0, 4), (quant_w1, 0, 5), (quant_x, 0, 5)] + steps(product, (0, 2), (0, 3), (1, 2), (1, 3))
+        vector_q += [(quant_w1, 0, 2), (quant_x, 0, 2), (quant_w1, 0, 3), (quant_x, 0, 3), (quant_w1, 0, 0), (quant_x, 0, 0), (quant_w1, 0, 1), (quant_x, 0, 1)]
+        vector_q += steps(product, (2, 4), (2, 5), (2, 2)) + [(quant_w1, 1, 4), (product, 2, 3)]
+        vector_q += [(quant_w1, 1, 5), (quant_x, 1, 4), by("vector", 1, 0, 20), (quant_x, 1, 2), (quant_x, 1, 0), (quant_w1, 1, 0), by("vector", 1, 1), by("vector", 1, 3, 0, 32), (quant_w1, 1, 2), (quant_w1, 1, 3), (quant_w1, 1, 1)]
+        vector_q += steps(product, (3, 4), (3, 5), (3, 2), (3, 3))
+        vector_q += [(quant_w2, 0, 0, KP), (quant_w2, 1, 0, KP), (weave_w2, 1, KP, SPLIT, "vector", 0, 32), (quant_w2, 0, KP, SPLIT), (weave_h, FRONT_A, 1, "vector"), (quant_w2, 1, KP, SPLIT), (quant_h, FRONT_A, 0), (quant_h, FRONT_A, 1), (quant_x, 2, 4), (quant_x, 2, 2), (quant_x, 2, 0), (quant_h, FRONT_B, 0)]
 
-        vector_q = [(widen, 1, 4, "vector"), by("vector", first, 0, HEAD_RUNS), (product, 0, 4), (quant_w1, first), (product, 0, 5), (product, 1, 4), (product, 1, 5)]
-        vector_q += [(quant_x, front(4)), (quant_w1, shared(0, 5)), (quant_x, front(5))]
-        vector_q += empties(front(2)) + [(quant_x, front(0)), (quant_w1, whole(0, 0)), (quant_x, front(2)), (quant_w1, shared(0, 2))]
-        vector_q += empties(front(3)) + [(quant_x, front(1)), (quant_w1, whole(0, 1)), (quant_x, front(3)), (quant_w1, shared(0, 3))]
-        vector_q += empties((2, 4)) + [(quant_w1, whole(1, 4)), (quant_x, (2, 4)), (quant_w1, shared(1, 5))]
-        vector_q += empties((2, 2)) + [(quant_w1, whole(1, 0)), (quant_x, (2, 2)), (quant_x, (2, 0)), by("vector", whole(1, 1))]
-        vector_q += [(quant_w1, whole(1, 2)), (quant_w1, shared(1, 3)), (quant_w1, whole(1, 1))]
-        vector_q += empties((3, 4)) + [(weave_w2, W2_PIECES[2], "vector"), (quant_x, (3, 4))]
-        vector_q += [(quant_h, FRONT_A, 0), (quant_w2, W2_PIECES[0]), (quant_w2, W2_PIECES[3]), (quant_w2, W2_PIECES[1]), (quant_w2, W2_PIECES[2])] + empties((3, 2))
-        vector_q += [(quant_h, FRONT_A, 1), (quant_x, (3, 2)), (quant_x, (3, 0)), (quant_h, FRONT_B, 0)]
-
-        after_root = [[(weave_h, THIRD, 0, "scalar")], [(relu, LAST, 0, 0), (weave_h, THIRD, 1, "scalar")],
-                      [(relu, LAST, 0, 2)], [(weave_h, LAST, 0, "scalar")],
-                      relus(LAST_A, 1) + [(weave_h, LAST_A, 1, "scalar")], relus(LAST_B, 1), [], []]
-        for n in range(NT):
-            scalar_q += [(root, n)] + after_root[n]
+        after_root = [[(weave_h, THIRD, 0, "scalar")], [(weave_h, THIRD, 1, "scalar")] + relus(LAST, 0, (0, 1)), relus(LAST, 0, (2, 3)),
+                      [(weave_h, LAST, 0, "scalar")], relus(LAST_A, 1) + [(relu_woven, LAST_B, 1, 0)], [(relu_woven, LAST_B, 1, t) for t in SL[1:]], []]
+        for n in range(NT - 1):
+            scalar_q += [(root, n, 0, L)] + after_root[n]
+        scalar_q += [(root,) + part for part in halves]
         after_tile = [[(quant_h, FRONT_B, 1)], [(quant_h, THIRD, 0)], [(quant_h, THIRD, 1)], [], [(quant_h, LAST, 0)]]
         for n in range(NT - 3):
-            vector_q += [(bias_wide, n)] + ([(noise, n - 1)] if n else []) + [(bias_narrow, n)]
-            vector_q += ([(shift, n - 1)] if n else []) + after_tile[n]
-        vector_q += [(bias_wide, 5), (noise, 4), (bias_narrow, 5), (shift, 4), (quant_h, LAST_A, 1), (noise, 5), (bias_wide, 6), (weave_h, LAST_B, 1, "vector"), (shift, 5), (quant_h, LAST_B, 1)]
-        vector_q += [(bias_narrow, 6), (noise, 6), (bias_wide, 7), (shift, 6), (bias_narrow, 7)]
+            vector_q += [wide(n)] + ([(noise, n - 1, 0, L)] if n else []) + [narrow(n)]
+            vector_q += ([(shift, n - 1, 0, L)] if n else []) + after_tile[n]
+        vector_q += [wide(5), (noise, 4, 0, L), (weave_h, LAST_A, 1, "vector"), narrow(5), (quant_h, LAST_A, 1), (shift, 4, 0, L), (noise, 5, 0, L), wide(6), (shift, 5, 0, L), (quant_h, LAST_B, 1)]
+        vector_q += [narrow(6), (noise, 6, 0, L)] + [(bias, NT - 1) + part for part in LAST_BIAS[:2]] + [(shift, 6, 0, L)] + [(bias, NT - 1) + part for part in LAST_BIAS[2:]]
         vector_q += [(f,) + part for f in (noise, shift) for part in halves]
-        tensor_q += [(fill_bank, LAST, 0, 0), (heads, 2), (fill_bank, LAST, 0, 2), (heads, 3), (heads, 4), (fill_bank, LAST_A, 1, 0), (heads, 5)]
-        tensor_q += [(fill_bank, LAST_B, 1, 0), (heads, NT - 2), (heads, NT - 1, FIRST_PASS), (heads, NT - 1, SECOND_PASS)]
-        behind = {(widen, 1, 4, "vector"): [(widen, 0, 4, "scalar")]}
 
-        everything = sync_q + tensor_q + scalar_q + vector_q + gpsimd_q
-        weaver = {step[1:-1]: step for step in everything if step[0] in (weave_w2, weave_h)}
-        widener = {step[1:-1]: step for step in everything if step[0] == widen}
-
-        widener.update({(2 * step[1] + i, step[2]): step for step in everything if step[0] == widen_both for i in range(2)})
-
-        def w1_steps(f, half, g):
-            return [step for step in everything if step[0] == f and step[1][:2] == (half, g)]
-
-        def emptier(q, g):
-            return (drain if g < STATE_PASSES else product, q, g)
-
-        def needs(f, *a):
-            if f == widen:
-                return [(load_obs, a[0] // 2, a[1])]
-            if f == widen_both:
-                return [(load_obs,) + a]
-            if f == turn:
-                q, g = a
-                if g < STATE_PASSES:
-                    return [(load_state, q, g if q in GROUPS[0] else 0)]
-                tiles = (2 * q, 2 * q + 1)
-                return [widener[n, g - g % 2] for n in tiles] + [(load_action, n) for n in tiles if g < STATE_PASSES + 2]
-            if f == product:
-                return [(turn,) + a, (load_scales,)]
-            if f == quant_x:
-                return [emptier(*key) for key in banks_of(a[0])]
-            if f in (weave_w1, pass_w1):
-                return [(load_w1,) + a[0][:2]]
-            if f == drain_w1:
-                return [(pass_w1,) + a]
-            if f == quant_w1:
-                return [step for step in everything if step[0] in (weave_w1, drain_w1) and step[1] == a[0]]
-            if f == first_pass:
-                return w1_steps(quant_w1, 0, ORDER[0][0]) + [(quant_first,) + a]
-            if f == quant_first:
-                return [emptier(a[0], ORDER[0][0])]
-            if f == front_pass:
-                return w1_steps(quant_w1, *a[:2]) + [(quant_x, ("front", a[1])) if a[1] != ORDER[0][0] or (quant_first, 1) not in everything else (quant_first, 1)]
-            if f == fill_bank:
-                quarter = GROUPS[a[0][0]][0]
-                return [s for g in range(G1) for s in w1_steps(quant_w1, a[1], g) + [(quant_x, pair_of(quarter, g)[0])]]
-            if f == relu:
-                span, half, t0 = a
-                if span != FRONT:
-                    return [(load_b1,), (fill_bank, span, half, bank_start(span, t0))]
-                last = [s for s in everything if s[:3] == (front_pass, half, ORDER[half][-1])]
-                return [(load_b1,)] + [s for s in last if len(s) == 3 or s[3] == t0]
-            if f == heads:
-                passes = a[1] if len(a) > 1 else ALL_PASSES
-                pieces = [(quant_h, span, half) for span, half in spans_of(a[0]) if half in passes]
-                return pieces + [(quant_w2, piece) for piece in W2_PIECES]
-            if f == bias_wide:
-                return [(heads, a[0], SECOND_PASS) if a[0] == NT - 1 else (heads, a[0]), (load_b2,)]
-            if f == weave_h:
-                return relus(FRONT if a[0][0] == 0 else a[0], a[1])
-            if f in (quant_w2, quant_h):
-                return [weaver[a]]
-            simple = {drain: [(turn,) + a], weave_w2: [(load_w2,) + a[:1]], bias_narrow: [(bias_wide,) + a],
-                      root: [(bias_wide,) + a], noise: [(root,) + a[:1], (load_eps,)],
-                      shift: [(noise,) + a, (bias_narrow,) + a[:1]], store_std: [(bias_wide,) + a],
-                      store_mean: [(bias_narrow,) + a], store_sample: [(shift,) + a]}
-            return simple.get(f, [])
-
-        def takes(f, *a):
-            if f == load_w1:
-                return [("wraw", DEPTH["wraw"], w1_steps(weave_w1, *a) + w1_steps(pass_w1, *a))]
-            if f == load_w2:
-                return [("wraw", DEPTH["wraw"], [weaver[a]])]
-            if f == load_obs:
-                return [("obs%d" % a[1], DEPTH["obs%d" % a[1]], [widener[2 * a[0] + i, a[1]] for i in range(2)])]
-            if f == load_state:
-                n = 1 if a[0] in GROUPS[0] else STATE_PASSES
-                return [("state%d" % n, DEPTH["state%d" % n], [(turn, a[0], a[1] + j) for j in range(n)])]
-            if f == widen_both:
-                return [("wide4", DEPTH["wide4"], [(turn, a[0], 4), (turn, a[0], 5)])]
-            if f in (load_action, widen):
-                n, g = a[0], a[1] if f == widen else STATE_PASSES
-                tag = "wide%d" % g
-                return [] if (n, g) in rows else [(tag, DEPTH[tag], [(turn, n // 2, g), (turn, n // 2, g + 1)])]
-            if f == weave_w1:
-                return [] if a[0] in woven else [(a[0][4], DEPTH[a[0][4]], [(quant_w1, a[0])])]
-            if f == pass_w1:
-                return [("tp", 4, [(drain_w1,) + a])]
-            if f == drain_w1:
-                return [] if a[1] else [(a[0][4], DEPTH[a[0][4]], [(quant_w1, a[0])])]
-            if f in (weave_w2, weave_h):
-                tag = weave_tag(a[-1])
-                return [(tag, DEPTH[tag], [(quant_w2 if f == weave_w2 else quant_h,) + a[:-1]])]
-            if f in (drain, product):
-                pair = pair_of(*a)[0]
-                return [] if ("x", pair) in woven else [("woven_x", DEPTH["woven_x"], [(quant_x, pair) if pair != ("front", ORDER[0][0]) or (quant_first, 1) not in everything else (quant_first, 1)])]
-            if f == turn:
-                return [(turn_tag(*a), 4, [emptier(*a)])]
-            if f == first_pass and a[0] == 0:
-                return [("acc", 4, [(relu, FRONT, 0, t - t % 2)]) for t in range(4)]
-            if f == front_pass and a[1] == ORDER[a[0]][0]:
-                return [("acc", 4, [(relu, FRONT, a[0], t - t % 2)]) for t in range(*(a[2:] or (4,)))]
-            if f == fill_bank:
-                return [(bank_tag(a[0], a[1]), 4, [(relu, a[0], a[1], a[2] + KP // a[0][2] - 2)])]
-            if f == relu and a[2] == 0:
-                return [(("hidden", a[0][2]), HIDDEN_DEPTH[a[0][2]], [s for k, s in weaver.items() if k == a[:2] or (a[0] == FRONT and k[0][0] == 0 and len(k) == 2 and k[1] == a[1])])]
-            if f == heads and a[1:] != (SECOND_PASS,):
-                return [("tp", 4, [(bias_wide, a[0])]), ("tp", 4, [(bias_narrow, a[0])])]
-            if f == bias_wide:
-                stores = [s for s in sync_q if s[0] in (store_std, store_mean, store_sample) and s[1] == a[0]]
-                return [("res", DEPTH["res"], stores)]
-            return []
+        in_bank = {}
+        for step in tensor_q:
+            if step[0] == mm1:
+                for t, g in pairs_of(*step[3:]):
+                    in_bank.setdefault(sums(step[1], step[2], t)[0], []).append((t, g))
 
         nc.vector.memset(ones[:], 1.0)
         make_identity(nc, ident[:])
-        make_identity(nc, ident_bf[:])
         nc.scalar.activation(scale_mixed[:ACTION_ROWS, :], ones[:], ACT.Sqrt)
 
-        done, held = set(), {}
         queues = [sync_q, tensor_q, scalar_q, vector_q, gpsimd_q]
+        def holder(key):
+            part_of = {"biased": "res", "root": "sample", "noise": "sample", "shifted": "sample"}
+            return (part_of[key[0]], key[1]) if key[0] in part_of else key
+
+        writers, users = {}, {}
+        for step in [step for queue in queues for step in queue]:
+            reads, writes = touches(*step)
+            for key in writes:
+                writers.setdefault(key, []).append(step)
+            for key in reads + writes:
+                users.setdefault(holder(key), []).append(step)
+        done = set()
         while any(queues):
             moved = False
             for queue in queues:
-                if not queue or not all(other in done for other in needs(*queue[0]) + behind.get(queue[0], [])):
+                if not queue:
                     continue
-                slots = takes(*queue[0])
-                taken = {tag: list(held.get(tag, [])) for tag, depth, readers in slots}
-                free = True
-                for tag, depth, readers in slots:
-                    previous = taken[tag][-depth] if len(taken[tag]) >= depth else []
-                    free = free and all(other in done for other in previous)
-                    taken[tag].append(readers)
-                if free:
-                    held.update(taken)
+                reads, writes = touches(*queue[0])
+                waits = [s for key in reads for s in writers.get(key, [])]
+                waits += [s for key in writes if key in before for s in users[before[key]]]
+                if all(s in done for s in waits):
                     step = queue.pop(0)
                     step[0](*step[1:])
                     done.add(step)

@@ -35,7 +35,7 @@ THIRD, LAST, LAST_A, LAST_B = (1, 0, QT), (2, 0, QT), (2, 0, P), (2, P, P)
 W2_PIECES = tuple((g, c0, min(KP, 2 * L - c0)) for g in range(G2) for c0 in (0, KP))
 H_PIECES = ((FRONT_A, 0), (FRONT_B, 0), (FRONT_A, 1), (FRONT_B, 1), (THIRD, 0), (THIRD, 1), (LAST, 0), (LAST_A, 1), (LAST_B, 1))
 CUT = 2 * KP - A
-OBS_LOADS = ((0, 1, CUT, O), (1, 1, CUT, O), (2, 2, CUT, O), (0, 2, 0, CUT), (2, 2, 0, CUT), (4, 2, 0, O), (6, 2, 0, O))
+OBS_LOADS = ((0, 1, CUT, CUT + KP), (1, 1, CUT, CUT + KP), (0, 2, CUT + KP, O), (2, 2, CUT, O), (0, 2, 0, CUT), (2, 2, 0, CUT), (4, 2, 0, O), (6, 2, 0, O))
 
 
 def rotate(keys, depth):
@@ -50,40 +50,44 @@ def w(*pairs):
     return [("w",) + pair for pair in pairs]
 
 
-W1_LOADS = [(0, 4), (0, 5), (0, 2), (0, 3), (0, 0), (0, 1), (1, 4), (1, 5), (1, 0), (1, 1), (1, 2), (1, 3)]
+W1_LOADS = [(0, 4), (0, 5), (0, 2), (0, 0), (0, 3), (0, 1), (1, 4), (1, 5), (1, 0), (1, 1), (1, 2), (1, 3)]
 HEADS = rotate([("head", n, c0) for n in range(NT) for c0 in (SPLIT, 0)], 4)
 BANKS = [
-    turned((0, 4), (0, 2), (0, 0), (2, 4), (2, 0)) + [("acc", THIRD, 0, 0)] + turned((3, 3)) + [("acc", THIRD, 1, 0), ("acc", LAST, 0, 2), ("acc", LAST_B, 1, 1)],
-    turned((0, 5), (0, 3), (0, 1), (2, 5), (2, 1), (3, 2), (3, 1)) + [("acc", LAST, 0, 0), ("acc", LAST_B, 1, 0)],
-    turned((1, 4), (1, 2), (1, 0), (2, 2), (3, 4)) + [("acc", THIRD, 0, 2), ("acc", THIRD, 1, 2), ("acc", LAST_B, 1, 2)],
-    turned((1, 5), (1, 3), (1, 1), (2, 3), (3, 5), (3, 0)) + [("acc", LAST_A, 1, 0), ("acc", LAST_B, 1, 3)],
-] + [[("acc", FRONT, 0, t), ("acc", FRONT, 1, t)] + HEADS[t] for t in range(4)]
+    turned((0, 4), (0, 2), (0, 0), (1, 0), (2, 2)) + [("acc", THIRD, 0, 0)] + turned((3, 2)) + [("acc", THIRD, 1, 0), ("acc", LAST, 0, 2), ("acc", LAST_B, 1, 1)],
+    turned((0, 5), (1, 2), (0, 1), (1, 1), (2, 3)) + [("acc", THIRD, 0, 2)] + turned((3, 3)) + [("acc", THIRD, 1, 2), ("acc", LAST_B, 1, 2)],
+    turned((1, 4), (0, 3), (2, 4), (2, 0), (3, 4), (3, 0)) + [("acc", LAST, 0, 0), ("acc", LAST_B, 1, 0)],
+    turned((1, 5), (1, 3), (2, 5), (2, 1), (3, 5), (3, 1)) + [("acc", LAST_A, 1, 0), ("acc", LAST_B, 1, 3)],
+] + [[("pass", 0, 5, t - 2)] * (t >= 2) + [("acc", FRONT, 0, t), ("acc", FRONT, 1, t)] + HEADS[t] for t in range(4)]
 WOVEN_LISTS = [
-    w((0, 5), (0, 3), (1, 0)) + [("w2", 1, 0)],
-    w((0, 4), (0, 1), (1, 5), (1, 3)) + [("w2", 0, 0)],
-    w((0, 2), (1, 4), (1, 2)),
-    w((0, 0), (1, 1)) + [("w2", 1, KP)],
+    w((0, 5), (0, 2), (0, 3), (1, 4), (1, 5), (1, 3)) + [("w2", 0, 0)],
+    w((0, 4), (1, 0)) + [("w2", 1, 0)],
+    w((0, 0), (0, 1), (1, 2)),
+    w((1, 1)) + [("w2", 1, KP)],
 ]
-NARROW_LISTS = rotate([("h", FRONT_A, 0), ("h", FRONT_B, 0), ("w2", 0, KP), ("h", FRONT_A, 1), ("h", FRONT_B, 1),
-                       ("h", THIRD, 0), ("h", THIRD, 1), ("h", LAST, 0), ("h", LAST_A, 1), ("h", LAST_B, 1)], 4)
+NARROW_LISTS = rotate([("w2", 0, KP), ("h", FRONT_A, 0), ("h", FRONT_A, 1), ("h", FRONT_B, 0), ("h", FRONT_B, 1),
+                       ("h", THIRD, 1), ("h", LAST, 0), ("h", LAST_A, 1), ("h", LAST_B, 1)], 4)
 SLICES_A_BANK = {FRONT: 1, THIRD: 2, LAST: 2, LAST_A: 4, LAST_B: 1}
-LAST_BIAS = ((L, L + L // 2), (L + L // 2, 2 * L), (0, SPLIT), (SPLIT, L))
+PIECE = 64
+POOL_COLS = 5 * PIECE
+X_LISTS = rotate([("x", 0, g) for g in (4, 5, 2, 3, 0, 1)] + [("x", grp, g) for grp in (1, 2) for g in (4, 2, 0)], 4)
+X_LISTS = X_LISTS[:2] + [X_LISTS[2] + [("h", THIRD, 0)], X_LISTS[3]]
 BUFFERS = {
     "bank": ("psum", [P, KP], F32, BANKS),
     "obs": ("keep", [P, 2 * O], U8, [[("obs", 0, CUT), ("obs", 4, 0)], [("obs", 1, CUT), ("obs", 6, 0)]]),
+    "obs_second": ("keep", [P, 2 * KP], U8, [[("obs", 0, CUT + KP)]]),
     "obs_front": ("keep", [P, 4 * KP], U8, [[("obs", 2, CUT)], [("obs", 0, 0)], [("obs", 2, 0)]]),
     "wide": ("keep", [P, 4 * KP], BF16, [[("wide", q, g), ("wide", q + 2, g)] for q in range(2) for g in (MIXED, LATE)]),
-    "state": ("keep", [P, 2, S], BF16, rotate([("state", q) for q in range(4)], 3)),
+    "state": ("keep", [P, 2, S], BF16, rotate([("state", q) for q in range(4)], 2)),
     "raw": ("keep", [P, 4, KP], BF16, rotate([("raw",) + key for key in W1_LOADS], 6)),
     "raw2": ("keep", [P, 4, 2 * L], BF16, rotate([("raw2", g) for g in range(G2)], 2)),
     "woven": ("keep", [P, WOVEN], BF16, WOVEN_LISTS),
     "narrow": ("keep", [P, WOVEN // 2], BF16, NARROW_LISTS),
-    "woven_x": ("keep", [P, WOVEN], BF16, rotate([("x", 0, g) for g in (4, 5, 2, 3, 0, 1)] + [("x", grp, g) for grp in (1, 2) for g in (4, 2, 0)], 4)),
+    "woven_x": ("keep", [P, WOVEN], BF16, X_LISTS),
     "hidden": ("keep", [P, WOVEN], BF16, [[("hidden", FRONT, half)] for half in range(2)]),
     "hidden_late": ("keep", [P, WOVEN // 2], BF16, rotate([("hidden", THIRD, 0), ("hidden", THIRD, 1), ("hidden", LAST, 0),
                                                            ("hidden", LAST_A, 1)], 3)),
-    "res": ("keep", [P, 2 * L], F32, rotate([("res", n) for n in range(NT)], 4)),
-    "sample": ("keep", [P, L], F32, rotate([("sample", n) for n in range(NT)], 4)),
+    "res": ("keep", [P, 2, 2 * L], F32, rotate([("res", n) for n in range(NT // 2)], 2)),
+    "sample": ("keep", [P, 2, L], F32, rotate([("sample", n) for n in range(NT // 2)], 3)),
 }
 
 
@@ -121,6 +125,7 @@ def tile_rssm_pa_kernel(tc, prev_state, prev_action, obs_bytes, obs_scale, eps,
         b2_rows = keep.tile([P, 2 * L], BF16)
         eps_sb = keep.tile([P, NT, L], BF16)
         ident = keep.tile([P, P], F32)
+        ident_bf = keep.tile([P, P], BF16)
 
         tile_of, before = {}, {}
         for family, (pool_name, shape, dtype, lists) in BUFFERS.items():
@@ -157,15 +162,14 @@ def tile_rssm_pa_kernel(tc, prev_state, prev_action, obs_bytes, obs_scale, eps,
         def load_state(q):
             nc.sync.dma_start(out=tile_of["state", q][:], in_=state_v[:, 2 * q:2 * q + 2, :])
 
-        def obs_cols(g):
-            return max(KP * g - S - A, 0), KP * (g + 2) - S - A
+        def obs_cols(g, passes):
+            return max(KP * g - S - A, 0), KP * (g + passes) - S - A
 
         def load_obs(n0, tiles, c0, c1):
             nc.sync.dma_start(out=tile_of["obs", n0, c0][:, :tiles * (c1 - c0)].rearrange("p (i c) -> p i c", i=tiles),
                               in_=bytes_v[:, n0:n0 + tiles, c0:c1])
 
-        def obs_load_of(n, g):
-            c0, c1 = obs_cols(g)
+        def obs_load_of(n, c0, c1):
             return [a for a in OBS_LOADS if a[0] <= n < a[0] + a[1] and a[2] <= c0 and c1 <= a[3]][0]
 
         def load_action(q):
@@ -181,12 +185,12 @@ def tile_rssm_pa_kernel(tc, prev_state, prev_action, obs_bytes, obs_scale, eps,
         def load_eps():
             nc.sync.dma_start(out=eps_sb[:], in_=eps_v)
 
-        def widen(n, g, engine):
-            c0, c1 = obs_cols(g)
-            n0, tiles, l0, l1 = obs_load_of(n, g)
+        def widen(n, g, passes, engine):
+            c0, c1 = obs_cols(g, passes)
+            n0, tiles, l0, l1 = obs_load_of(n, c0, c1)
             at = (n - n0) * (l1 - l0) + c0 - l0
-            end = 2 * KP * (n % 2 + 1)
-            copy[engine](out=tile_of["wide", n // 2, g][:, end - (c1 - c0):end],
+            end = 2 * KP * (n % 2) + KP * (g % 2 + passes)
+            copy[engine](out=tile_of["wide", n // 2, g - g % 2][:, end - (c1 - c0):end],
                          in_=tile_of["obs", n0, l0][:, at:at + c1 - c0].bitcast(FP8))
 
         def rows(n, g):
@@ -234,6 +238,18 @@ def tile_rssm_pa_kernel(tc, prev_state, prev_action, obs_bytes, obs_scale, eps,
                 copy[engine](out=woven.rearrange("p (s r e t) -> p r t e s", r=RUNS, e=2, t=4)[:, r0:r1],
                              in_=raw.rearrange("p t (r e s) -> p r t e s", e=2, s=4)[:, r0:r1])
 
+        def pass_w1(half, g, k):
+            bank = tile_of["pass", half, g, k][:].bitcast(BF16).rearrange("p (c u e) -> p c u e", u=2, e=2)
+            cols = tile_of["raw", half, g][:, :, QT * k:QT * (k + 1)]
+            for u in range(2):
+                nc.tensor.matmul(bank[:, :, u, :], ident_bf[:], cols[:, 2 * u:2 * u + 2, :].rearrange("p e c -> p c e"),
+                                 start=True, stop=True)
+
+        def drain_w1(half, g, k):
+            m0 = QT * k // 4
+            out = tile_of["w", half, g][:].bitcast(F32).rearrange("p (s m v) -> p m s v", s=4, v=2)[:, m0:m0 + QT // 4]
+            nc.scalar.copy(out=out, in_=tile_of["pass", half, g, k][:].rearrange("p (m s v) -> p m s v", s=4, v=2))
+
         def quant_w1(half, g):
             cols = slice(KP * half, KP * half + KP)
             nc.vector.quantize_mx(out=w1c[:, g, cols].bitcast(FP8X4), scales=w1s[:, g, cols], in_=tile_of["w", half, g][:])
@@ -275,11 +291,15 @@ def tile_rssm_pa_kernel(tc, prev_state, prev_action, obs_bytes, obs_scale, eps,
             nc.scalar.activation(tile_of["hidden", span, half][:, n * t:n * t + n], tile_of[key][:, at:at + n], ACT.Relu,
                                  bias=b1_cols[:, half, t:t + 1])
 
-        def relu_woven(span, half, t):
+        def relu_woven(span, half, t, engine):
             key, at = sums(span, half, t)
             n = span[2]
             out = tile_of["h", span, half][:, :4 * n].rearrange("p (n t) -> p n t", t=4)[:, :, t]
-            nc.scalar.activation(out, tile_of[key][:, at:at + n], ACT.Relu, bias=b1_cols[:, half, t:t + 1])
+            if engine == "scalar":
+                nc.scalar.activation(out, tile_of[key][:, at:at + n], ACT.Relu, bias=b1_cols[:, half, t:t + 1])
+            else:
+                nc.vector.tensor_scalar(out=out, in0=tile_of[key][:, at:at + n], scalar1=b1_cols[:, half, t:t + 1], scalar2=0.0,
+                                        op0=ALU.add, op1=ALU.max)
 
         def parent(span):
             return FRONT if span[0] == 0 else span
@@ -307,42 +327,50 @@ def tile_rssm_pa_kernel(tc, prev_state, prev_action, obs_bytes, obs_scale, eps,
                                         lhsT_scale=hs[grp][:, g, r0:r0 + P], rhs=w2c[:, g, c0:c1].bitcast(FP8X4),
                                         rhs_scale=w2s[:, g, c0:c1], start=(g == 0), stop=(g == G2 - 1))
 
-        def bias_parts(n):
-            return LAST_BIAS if n == NT - 1 else ((SPLIT, 2 * L), (0, SPLIT))
+        def res(n):
+            return tile_of["res", n // 2][:, n % 2, :]
+
+        def both(kind, n, tiles, c0, c1):
+            return tile_of[kind, n // 2][:, n % 2:n % 2 + tiles, c0:c1]
 
         def bias(n, c0, c1):
-            b0 = SPLIT if c0 >= SPLIT else 0
-            nc.vector.tensor_add(out=tile_of["res", n][:, c0:c1], in0=tile_of["head", n, b0][:, c0 - b0:c1 - b0], in1=b2_rows[:, c0:c1])
+            b0 = SPLIT * (c0 >= SPLIT)
+            nc.vector.tensor_add(out=res(n)[:, c0:c1], in0=tile_of["head", n, b0][:, c0 - b0:c1 - b0], in1=b2_rows[:, c0:c1])
 
         def root(n, c0, c1):
-            nc.scalar.activation(tile_of["sample", n][:, c0:c1], tile_of["res", n][:, L + c0:L + c1], ACT.Sqrt)
+            nc.scalar.activation(tile_of["sample", n // 2][:, n % 2, c0:c1], res(n)[:, L + c0:L + c1], ACT.Sqrt)
 
-        def noise(n, c0, c1):
-            part = tile_of["sample", n][:, c0:c1]
-            nc.vector.tensor_mul(out=part, in0=part, in1=eps_sb[:, n, c0:c1])
+        def noise(n, tiles, c0, c1):
+            part = both("sample", n, tiles, c0, c1)
+            nc.vector.tensor_mul(out=part, in0=part, in1=eps_sb[:, n:n + tiles, c0:c1])
 
-        def shift(n, c0, c1):
-            part = tile_of["sample", n][:, c0:c1]
-            nc.vector.tensor_add(out=part, in0=part, in1=tile_of["res", n][:, c0:c1])
+        def shift(n, tiles, c0, c1, engine):
+            part = both("sample", n, tiles, c0, c1)
+            add = nc.gpsimd.tensor_add if engine == "gpsimd" else nc.vector.tensor_add
+            add(out=part, in0=part, in1=both("res", n, tiles, c0, c1))
 
-        def store_std(n, c0, c1):
-            nc.sync.dma_start(out=std_v[:, n, c0:c1], in_=tile_of["res", n][:, L + c0:L + c1])
+        def store_std(n):
+            nc.sync.dma_start(out=std_v[:, n, :], in_=res(n)[:, L:])
 
         def store_mean(n):
-            nc.sync.dma_start(out=mean_v[:, n, :], in_=tile_of["res", n][:, :L])
+            nc.sync.dma_start(out=mean_v[:, n, :], in_=res(n)[:, :L])
 
-        def store_sample(n, c0, c1):
-            nc.sync.dma_start(out=sample_v[:, n, c0:c1], in_=tile_of["sample", n][:, c0:c1])
+        def store_sample(n, tiles, c0, c1):
+            nc.sync.dma_start(out=sample_v[:, n:n + tiles, c0:c1], in_=both("sample", n, tiles, c0, c1))
+
+        def parts(kind, n, tiles, c0, c1):
+            return [(kind, n + i, c) for i in range(tiles) for c in range(c0, c1, PIECE)]
 
         def touches(f, *a):
             if f == load_obs:
                 return [], [("obs", a[0], a[2])]
             if f == widen:
-                load = obs_load_of(*a[:2])
-                return [("obs", load[0], load[2])], [("wide", a[0] // 2, a[1])]
+                n, g, passes = a[:3]
+                load = obs_load_of(n, *obs_cols(g, passes))
+                return [("obs", load[0], load[2])], [("wide", n // 2, g - g % 2)] + [("rows", n // 2, g + j) for j in range(passes)]
             if f == turn:
                 q, g = a
-                return [("state", q) if g < STATE_PASSES else ("wide", q, g - g % 2)], [("turn", q, g)]
+                return [("state", q) if g < STATE_PASSES else ("rows", q, g)], [("turn", q, g)]
             if f in (drain, product):
                 scales = [] if f == drain else ["mixed"] if a[1] == MIXED else ["scales"]
                 return [("turn",) + a] + scales, [x_key(*a)[0]]
@@ -353,17 +381,20 @@ def tile_rssm_pa_kernel(tc, prev_state, prev_action, obs_bytes, obs_scale, eps,
             if f == relu:
                 return [sums(*a)[0], "b1"], [("hidden",) + a[:2]]
             if f == relu_woven:
-                return [sums(*a)[0], "b1"], [("h",) + a[:2]]
+                return [sums(*a[:3])[0], "b1"], [("h",) + a[:2]]
             if f == bias:
-                n, c0, c1 = a
-                return [("head", n, SPLIT if c0 >= SPLIT else 0), "b2"], [("res", n), ("biased", n, c0)]
-            if f in (root, store_std):
-                n, c0, c1 = a
-                std = [("biased", n, b0) for b0, b1 in bias_parts(n) if b0 < L + c1 and L + c0 < b1]
-                return std, [("sample", n), ("root",) + a] if f == root else []
+                return [("head", a[0], SPLIT * (a[1] >= SPLIT)), "b2"], [("res", a[0] // 2)] + parts("biased", a[0], 1, a[1], a[2])
+            if f == root:
+                return parts("biased", a[0], 1, L + a[1], L + a[2]), [("sample", a[0] // 2)] + parts("root", a[0], 1, a[1], a[2])
             if f == noise:
-                n, c0, c1 = a
-                return [("root",) + a, "eps"], [("noise",) + a]
+                return parts("root", *a) + ["eps"], parts("noise", *a)
+            if f == shift:
+                return parts("noise", *a[:4]) + parts("biased", *a[:4]), parts("shifted", *a[:4])
+            if f in (store_std, store_mean):
+                c0 = L * (f == store_std)
+                return parts("biased", a[0], 1, c0, c0 + L), []
+            if f == store_sample:
+                return parts("shifted", *a), []
             if f == weave_h:
                 return [("hidden", parent(a[0]), a[1])], [("h",) + a[:2]]
             if f == heads:
@@ -374,14 +405,12 @@ def tile_rssm_pa_kernel(tc, prev_state, prev_action, obs_bytes, obs_scale, eps,
             return {load_scales: ([], ["scales"]), load_mixed_scales: ([], ["mixed"]), load_b1: ([], ["b1"]),
                     load_b2: ([], ["b2"]), load_eps: ([], ["eps"]),
                     load_w1: ([], [("raw",) + a]), load_w2: ([], [("raw2",) + a]), load_state: ([], [("state",) + a]),
-                    load_action: ([], [("wide",) + a + (MIXED,)]),
+                    load_action: ([], [("wide",) + a + (MIXED,), ("rows",) + a + (MIXED,)]),
                     quant_x: ([("x",) + a], [("xq",) + a]),
+                    pass_w1: ([("raw",) + a[:2]], [("pass",) + a]), drain_w1: ([("pass",) + a], [("w",) + a[:2]]),
                     weave_w1: ([("raw",) + a[:2]], [("w",) + a[:2]]), quant_w1: ([("w",) + a], [("wq",) + a]),
                     weave_w2: ([("raw2",) + a[:1]], [("w2",) + a[:2]]), quant_w2: ([("w2",) + a[:2]], [("w2q",) + a[:2]]),
-                    quant_h: ([("h",) + a], [("hq",) + a]),
-                    shift: ([("noise",) + a, ("res",) + a[:1]], [("shifted",) + a]),
-                    store_mean: ([("res",) + a], []),
-                    store_sample: ([("shifted",) + a, ("sample",) + a[:1]], [])}[f]
+                    quant_h: ([("h",) + a], [("hq",) + a])}[f]
 
         SL = (0, 1, 2, 3)
 
@@ -392,7 +421,7 @@ def tile_rssm_pa_kernel(tc, prev_state, prev_action, obs_bytes, obs_scale, eps,
             return [(f,) + a for a in args]
 
         def widens(q, g):
-            return [(widen, 2 * q, g, "scalar"), (widen, 2 * q + 1, g, "scalar")]
+            return [(widen, 2 * q, g, 2, "scalar"), (widen, 2 * q + 1, g, 2, "scalar")]
 
         def relus(span, half, slices=SL):
             return [(relu, span, half, t) for t in slices]
@@ -403,58 +432,63 @@ def tile_rssm_pa_kernel(tc, prev_state, prev_action, obs_bytes, obs_scale, eps,
         def narrow(n):
             return (bias, n, 0, SPLIT)
 
-        halves = [(NT - 1, 0, L // 2), (NT - 1, L // 2, L)]
-        stores = []
-        for n in range(NT):
-            earlier = [(store_sample, n - 1, 0, L)] if n else []
-            stores += [(store_std, n, 0, L)] + (earlier + [(store_mean, n)] if n >= NT - 2 else [(store_mean, n)] + earlier)
-        stores += [(store_sample,) + part for part in halves]
-
         obs = [(load_obs,) + a for a in OBS_LOADS]
         w1_loads = [(load_w1,) + key for key in W1_LOADS]
-        sync_q = obs[:2] + [(load_scales,), obs[2]] + w1_loads[:2] + [obs[3], (load_action, 0), w1_loads[2], obs[4], (load_action, 1), (load_mixed_scales,)]
-        sync_q += w1_loads[3:6] + [(load_state, 0), (load_state, 1), obs[5], (load_action, 2), (load_b1,)]
-        sync_q += [w1_loads[6], w1_loads[7], obs[6], (load_action, 3), w1_loads[8], (load_state, 2)] + w1_loads[9:] + [(load_w2, 0), (load_w2, 1), (load_state, 3), (load_b2,), (load_eps,)] + stores
+        stores = []
+        for n in range(NT):
+            earlier = [(store_sample, n - 1, 1, 0, L)] if n else []
+            stores += [(store_std, n)] + (earlier + [(store_mean, n)] if n >= NT - 2 else [(store_mean, n)] + earlier)
+        stores += steps(store_sample, (NT - 1, 1, 0, L // 2), (NT - 1, 1, L // 2, L))
+        sync_q = obs[:2] + [(load_scales,)] + obs[2:4] + w1_loads[:2] + [obs[4], (load_action, 0), obs[5], (load_action, 1), (load_mixed_scales,)]
+        sync_q += w1_loads[2:5] + [(load_state, 0), (load_state, 1), obs[6], (load_action, 2), w1_loads[5], (load_b1,)]
+        sync_q += [w1_loads[6], (load_state, 2), obs[7], (load_action, 3)] + w1_loads[7:] + [(load_w2, 0), (load_w2, 1), (load_state, 3), (load_b2,), (load_eps,)] + stores
 
         ALL = (4, 5, 2, 3, 0, 1)
-        tensor_q = steps(turn, (0, 4), (0, 5), (1, 4), (1, 5), (0, 2), (0, 3)) + [(mm1, FRONT, 0, SL, (4,))] + steps(turn, (1, 2), (1, 3)) + [(mm1, FRONT, 0, SL, (5,))]
-        tensor_q += steps(turn, (0, 0), (0, 1), (1, 0), (1, 1)) + [(mm1, FRONT, 0, SL, (2, 3))]
-        tensor_q += steps(turn, (2, 4), (2, 5)) + [(mm1, FRONT, 0, SL, (0,))] + steps(turn, (2, 2), (2, 3)) + [(mm1, FRONT, 0, SL, (1,))]
-        tensor_q += steps(turn, (2, 0), (2, 1)) + [(mm1, FRONT, 1, SL, (4, 5)), (mm1, THIRD, 0, (0, 1), ALL[:4]), (mm1, THIRD, 0, (0, 1), ALL[4:])] + steps(turn, (3, 4), (3, 5)) + [(mm1, FRONT, 1, SL, (0, 2, 3))]
-        tensor_q += steps(turn, (3, 2), (3, 3)) + [(mm1, FRONT, 1, SL, (1,)), (mm1, THIRD, 0, (2, 3), ALL)] + steps(turn, (3, 0), (3, 1))
+        tensor_q = steps(turn, (0, 4), (0, 5), (1, 4), (1, 5)) + steps(pass_w1, (0, 5, 0), (0, 5, 1)) + steps(turn, (0, 2), (0, 3)) + [(mm1, FRONT, 0, SL, (4,))]
+        tensor_q += steps(turn, (1, 2), (1, 3)) + [(mm1, FRONT, 0, SL, (5,))] + steps(turn, (0, 0), (0, 1)) + [(mm1, FRONT, 0, (0, 1), (2,))]
+        tensor_q += steps(turn, (1, 0), (1, 1)) + [(mm1, FRONT, 0, (2, 3), (2,))] + steps(turn, (2, 4), (2, 5)) + [(mm1, FRONT, 0, SL, (3,))]
+        tensor_q += steps(turn, (2, 2), (2, 3)) + [(mm1, FRONT, 0, SL, (0,))]
+        tensor_q += steps(turn, (2, 0), (2, 1)) + [(mm1, FRONT, 0, SL, (1,))] + steps(turn, (3, 4), (3, 5))
+        tensor_q += [(mm1, THIRD, 0, (0, 1), ALL[:2]), (mm1, FRONT, 1, SL, (4, 5)), (mm1, THIRD, 0, (0, 1), ALL[2:]), (mm1, THIRD, 0, (2, 3), ALL), (mm1, FRONT, 1, SL, (2, 0))]
+        tensor_q += steps(turn, (3, 2), (3, 3)) + [(mm1, FRONT, 1, SL, (3, 1))] + steps(turn, (3, 0), (3, 1))
         tensor_q += [(mm1, THIRD, 1, SL, ALL), (heads, 0, (0, 1)), (heads, 1, (0, 1)), (mm1, LAST, 0, (0, 1), ALL), (heads, 2, (0, 1))]
         tensor_q += [(mm1, LAST, 0, (2, 3), ALL), (heads, 3, (0, 1)), (heads, 4, (0, 1)), (mm1, LAST_A, 1, SL, ALL), (heads, 5, (0, 1))]
         tensor_q += [(mm1, LAST_B, 1, SL, ALL), (heads, 6, (0, 1)), (heads, 7, (0,)), (heads, 7, (1,))]
 
-        gpsimd_q = [by("gpsimd", 0, 4, 0, 36), by("gpsimd", 0, 5, 0, 44), by("gpsimd", 0, 3, 0, 30), by("gpsimd", 0, 2, 24), by("gpsimd", 0, 0, 40)]
-        gpsimd_q += [by("gpsimd", 1, 5), by("gpsimd", 1, 0, 0, 20), (weave_w2, 0, 0, KP, "gpsimd", 0, 64), (weave_w2, 0, KP, SPLIT, "gpsimd", 0, 32)]
+        gpsimd_q = [by("gpsimd", 0, 4, 0, 32), by("gpsimd", 0, 2, 0, 56), by("gpsimd", 0, 3, 0, 56)]
+        gpsimd_q += [by("gpsimd", 0, 1, 0, 54), by("gpsimd", 1, 5, 0, 56), (weave_w2, 0, 0, KP, "gpsimd", 0, 64), (weave_w2, 0, KP, SPLIT, "gpsimd", 0, 32), (weave_w2, 1, KP, SPLIT, "gpsimd", 0, 20)]
+        gpsimd_q += [(weave_h, THIRD, 0, "gpsimd")]
 
-        scalar_q = [(widen, 1, LATE, "scalar"), (widen, 3, LATE, "scalar"), by("scalar", 0, 4, 36), by("scalar", 0, 5, 44)]
-        scalar_q += widens(0, MIXED) + [by("scalar", 0, 2, 0, 24)] + widens(1, MIXED) + [by("scalar", 0, 3, 30), by("scalar", 0, 0, 0, 40), by("scalar", 0, 1)] + steps(drain, (0, 0), (0, 1), (1, 0), (1, 1))
-        scalar_q += widens(2, LATE) + widens(2, MIXED) + [by("scalar", 1, 4)] + relus(FRONT, 0) + steps(drain, (2, 0), (2, 1))
-        scalar_q += widens(3, LATE) + [by("scalar", 1, 2), by("scalar", 1, 3, 32)] + relus(THIRD, 0, (0, 1)) + widens(3, MIXED) + [(weave_w2, 1, 0, KP, "scalar", 0, 64)]
-        scalar_q += relus(FRONT, 1) + [(weave_h, FRONT_A, 0, "scalar")] + relus(THIRD, 0, (2, 3)) + steps(drain, (3, 0), (3, 1)) + [(weave_h, FRONT_B, 0, "scalar"), (weave_h, FRONT_B, 1, "scalar")] + relus(THIRD, 1)
+        scalar_q = [(widen, 1, LATE, 1, "scalar"), (widen, 0, LATE + 1, 1, "scalar"), (widen, 1, LATE + 1, 1, "scalar")] + widens(1, LATE) + [by("scalar", 0, 4, 32)]
+        scalar_q += widens(0, MIXED) + steps(drain_w1, (0, 5, 0), (0, 5, 1)) + widens(1, MIXED) + [by("scalar", 0, 2, 56), by("scalar", 0, 0), by("scalar", 0, 3, 56)] + steps(drain, (0, 0), (0, 1)) + widens(2, LATE) + steps(drain, (1, 0), (1, 1))
+        scalar_q += widens(2, MIXED) + [by("scalar", 0, 1, 54), by("scalar", 1, 4)] + widens(3, LATE) + steps(drain, (2, 0), (2, 1)) + [by("scalar", 1, 5, 56)] + relus(FRONT, 0)
+        scalar_q += [by("scalar", 1, 2), by("scalar", 1, 3, 20)] + relus(THIRD, 0, (0, 1)) + widens(3, MIXED) + relus(THIRD, 0, (2, 3)) + [(weave_w2, 1, 0, KP, "scalar", 0, 64), (weave_h, FRONT_A, 0, "scalar")]
+        scalar_q += relus(FRONT, 1) + [(weave_h, FRONT_A, 1, "scalar")] + steps(drain, (3, 0), (3, 1)) + [(weave_h, FRONT_B, 0, "scalar"), (weave_h, FRONT_B, 1, "scalar")]
 
-        vector_q = [(widen, 0, LATE, "vector"), (widen, 2, LATE, "vector")] + steps(product, (0, 4), (0, 5), (1, 4), (1, 5))
-        vector_q += [(quant_w1, 0, 4), (quant_x, 0, 4), (quant_w1, 0, 5), (quant_x, 0, 5)] + steps(product, (0, 2), (0, 3), (1, 2), (1, 3))
-        vector_q += [(quant_w1, 0, 2), (quant_x, 0, 2), (quant_w1, 0, 3), (quant_x, 0, 3), (quant_w1, 0, 0), (quant_x, 0, 0), (quant_w1, 0, 1), (quant_x, 0, 1)]
-        vector_q += steps(product, (2, 4), (2, 5), (2, 2)) + [(quant_w1, 1, 4), (product, 2, 3)]
-        vector_q += [(quant_w1, 1, 5), (quant_x, 1, 4), by("vector", 1, 0, 20), (quant_x, 1, 2), (quant_x, 1, 0), (quant_w1, 1, 0), by("vector", 1, 1), by("vector", 1, 3, 0, 32), (quant_w1, 1, 2), (quant_w1, 1, 3), (quant_w1, 1, 1)]
+        vector_q = [(widen, 0, LATE, 1, "vector")] + steps(product, (0, 4), (0, 5), (1, 4), (1, 5))
+        vector_q += [(quant_w1, 0, 4), (quant_x, 0, 4), (quant_w1, 0, 5), (quant_x, 0, 5)] + steps(product, (0, 2), (1, 2))
+        vector_q += [(quant_w1, 0, 2), (quant_x, 0, 2)] + steps(product, (0, 3), (1, 3)) + [(quant_w1, 0, 3), (quant_x, 0, 3), (quant_w1, 0, 0), (quant_x, 0, 0)]
+        vector_q += steps(product, (2, 4), (2, 5)) + [(quant_x, 0, 1), (quant_w1, 0, 1), (quant_w1, 1, 4), (quant_x, 1, 4)] + steps(product, (2, 2), (2, 3))
+        vector_q += [(quant_w1, 1, 5), (quant_x, 1, 2), (quant_x, 1, 0), by("vector", 1, 0), (quant_w1, 1, 2), (quant_w1, 1, 0), by("vector", 1, 3, 0, 20), by("vector", 1, 1), (quant_w1, 1, 3), (quant_w1, 1, 1)]
         vector_q += steps(product, (3, 4), (3, 5), (3, 2), (3, 3))
-        vector_q += [(quant_w2, 0, 0, KP), (quant_w2, 1, 0, KP), (weave_w2, 1, KP, SPLIT, "vector", 0, 32), (quant_w2, 0, KP, SPLIT), (weave_h, FRONT_A, 1, "vector"), (quant_w2, 1, KP, SPLIT), (quant_h, FRONT_A, 0), (quant_h, FRONT_A, 1), (quant_x, 2, 4), (quant_x, 2, 2), (quant_x, 2, 0), (quant_h, FRONT_B, 0)]
+        vector_q += [(quant_w2, 0, 0, KP), (quant_w2, 1, 0, KP), (weave_w2, 1, KP, SPLIT, "vector", 20, 32), (quant_w2, 0, KP, SPLIT), (quant_h, FRONT_A, 0), (quant_w2, 1, KP, SPLIT), (quant_x, 2, 4), (quant_h, FRONT_A, 1), (quant_x, 2, 2), (quant_x, 2, 0)]
 
-        after_root = [[(weave_h, THIRD, 0, "scalar")], [(weave_h, THIRD, 1, "scalar")] + relus(LAST, 0, (0, 1)), relus(LAST, 0, (2, 3)),
-                      [(weave_h, LAST, 0, "scalar")], relus(LAST_A, 1) + [(relu_woven, LAST_B, 1, 0)], [(relu_woven, LAST_B, 1, t) for t in SL[1:]], []]
-        for n in range(NT - 1):
-            scalar_q += [(root, n, 0, L)] + after_root[n]
-        scalar_q += [(root,) + part for part in halves]
-        after_tile = [[(quant_h, FRONT_B, 1)], [(quant_h, THIRD, 0)], [(quant_h, THIRD, 1)], [], [(quant_h, LAST, 0)]]
-        for n in range(NT - 3):
-            vector_q += [wide(n)] + ([(noise, n - 1, 0, L)] if n else []) + [narrow(n)]
-            vector_q += ([(shift, n - 1, 0, L)] if n else []) + after_tile[n]
-        vector_q += [wide(5), (noise, 4, 0, L), (weave_h, LAST_A, 1, "vector"), narrow(5), (quant_h, LAST_A, 1), (shift, 4, 0, L), (noise, 5, 0, L), wide(6), (shift, 5, 0, L), (quant_h, LAST_B, 1)]
-        vector_q += [narrow(6), (noise, 6, 0, L)] + [(bias, NT - 1) + part for part in LAST_BIAS[:2]] + [(shift, 6, 0, L)] + [(bias, NT - 1) + part for part in LAST_BIAS[2:]]
-        vector_q += [(f,) + part for f in (noise, shift) for part in halves]
+        def sample(n):
+            return [(noise, n, 1, 0, L), (shift, n, 1, 0, L, "vector")]
+
+        def rooted(n):
+            return (root, n, 0, L)
+
+        end, mid = NT - 1, L // 2
+        scalar_q += [rooted(0)] + relus(THIRD, 1, (0, 1)) + [rooted(1)] + relus(THIRD, 1, (2, 3)) + relus(LAST, 0, (0, 1)) + [(weave_h, THIRD, 1, "scalar"), rooted(2)] + relus(LAST, 0, (2, 3))
+        scalar_q += [rooted(3), (weave_h, LAST, 0, "scalar"), rooted(4)] + relus(LAST_A, 1) + [(weave_h, LAST_A, 1, "scalar"), (relu_woven, LAST_B, 1, 0, "scalar"), rooted(5)] + [(relu_woven, LAST_B, 1, t, "scalar") for t in SL[1:]] + [rooted(6), (root, end, 0, mid), (root, end, mid, L)]
+        vector_q += [wide(0), wide(1), narrow(0), narrow(1), (quant_h, FRONT_B, 0), (quant_h, FRONT_B, 1), sample(0)[0], (quant_h, THIRD, 0), sample(0)[1]]
+        vector_q += [sample(1)[0], wide(2), sample(1)[1], narrow(2), (quant_h, THIRD, 1)]
+        for n in (3, 4):
+            vector_q += [wide(n), sample(n - 1)[0], narrow(n), sample(n - 1)[1]]
+        vector_q += [(quant_h, LAST, 0), wide(5), sample(4)[0], narrow(5), (quant_h, LAST_A, 1), sample(4)[1], sample(5)[0], wide(6), sample(5)[1], (quant_h, LAST_B, 1), narrow(6)]
+        vector_q += [sample(6)[0], (bias, end, L, L + mid), (bias, end, L + mid, 2 * L), sample(6)[1], narrow(end), (bias, end, SPLIT, L)]
+        vector_q += [(noise, end, 1, 0, mid), (noise, end, 1, mid, L), (shift, end, 1, 0, mid, "vector"), (shift, end, 1, mid, L, "vector")]
 
         in_bank = {}
         for step in tensor_q:
@@ -464,12 +498,15 @@ def tile_rssm_pa_kernel(tc, prev_state, prev_action, obs_bytes, obs_scale, eps,
 
         nc.vector.memset(ones[:], 1.0)
         make_identity(nc, ident[:])
+        make_identity(nc, ident_bf[:])
         nc.scalar.activation(scale_mixed[:ACTION_ROWS, :], ones[:], ACT.Sqrt)
 
         queues = [sync_q, tensor_q, scalar_q, vector_q, gpsimd_q]
         def holder(key):
             part_of = {"biased": "res", "root": "sample", "noise": "sample", "shifted": "sample"}
-            return (part_of[key[0]], key[1]) if key[0] in part_of else key
+            if key[0] == "rows":
+                return ("wide", key[1], key[2] - key[2] % 2)
+            return (part_of[key[0]], key[1] // 2) if key[0] in part_of else key
 
         writers, users = {}, {}
         for step in [step for queue in queues for step in queue]:

@@ -57,20 +57,22 @@ BANKS = [
     turned((0, 5), (1, 2), (0, 1), (1, 1), (2, 3)) + [("acc", THIRD, 0, 2)] + turned((3, 3)) + [("acc", THIRD, 1, 2), ("acc", LAST_B, 1, 2)],
     turned((1, 4), (0, 3), (2, 4), (2, 0), (3, 4), (3, 0)) + [("acc", LAST, 0, 0), ("acc", LAST_B, 1, 0)],
     turned((1, 5), (1, 3), (2, 5), (2, 1), (3, 5), (3, 1)) + [("acc", LAST_A, 1, 0), ("acc", LAST_B, 1, 3)],
-] + [[("pass", 0, 5, t - 2)] * (t >= 2) + [("acc", FRONT, 0, t), ("acc", FRONT, 1, t)] + HEADS[t] for t in range(4)]
+] + [[("acc", FRONT, 0, t), ("acc", FRONT, 1, t)] + HEADS[t] for t in range(4)]
 WOVEN_LISTS = [
     w((0, 5), (0, 2), (0, 3), (1, 4), (1, 5), (1, 3)) + [("w2", 0, 0)],
-    w((0, 4), (1, 0)) + [("w2", 1, 0)],
-    w((0, 0), (0, 1), (1, 2)),
+    w((0, 4), (0, 0), (1, 0)) + [("w2", 1, 0)],
+    [("x", 0, 0)] + w((0, 1), (1, 2)) + [("x", 2, 2)],
     w((1, 1)) + [("w2", 1, KP)],
+    [("x", 0, 4), ("x", 0, 3), ("x", 1, 2), ("x", 2, 4)],
+    [("x", 0, 5), ("x", 0, 1), ("x", 2, 0), ("h", THIRD, 0)],
+    [("x", 0, 2), ("x", 1, 4)],
+    [("x", 1, 0)],
 ]
 NARROW_LISTS = rotate([("w2", 0, KP), ("h", FRONT_A, 0), ("h", FRONT_A, 1), ("h", FRONT_B, 0), ("h", FRONT_B, 1),
                        ("h", THIRD, 1), ("h", LAST, 0), ("h", LAST_A, 1), ("h", LAST_B, 1)], 4)
 SLICES_A_BANK = {FRONT: 1, THIRD: 2, LAST: 2, LAST_A: 4, LAST_B: 1}
 PIECE = 64
 POOL_COLS = 5 * PIECE
-X_LISTS = rotate([("x", 0, g) for g in (4, 5, 2, 3, 0, 1)] + [("x", grp, g) for grp in (1, 2) for g in (4, 2, 0)], 4)
-X_LISTS = X_LISTS[:2] + [X_LISTS[2] + [("h", THIRD, 0)], X_LISTS[3]]
 BUFFERS = {
     "bank": ("psum", [P, KP], F32, BANKS),
     "obs": ("keep", [P, 2 * O], U8, [[("obs", 0, CUT), ("obs", 4, 0)], [("obs", 1, CUT), ("obs", 6, 0)]]),
@@ -82,7 +84,6 @@ BUFFERS = {
     "raw2": ("keep", [P, 4, 2 * L], BF16, rotate([("raw2", g) for g in range(G2)], 2)),
     "woven": ("keep", [P, WOVEN], BF16, WOVEN_LISTS),
     "narrow": ("keep", [P, WOVEN // 2], BF16, NARROW_LISTS),
-    "woven_x": ("keep", [P, WOVEN], BF16, X_LISTS),
     "hidden": ("keep", [P, WOVEN], BF16, [[("hidden", FRONT, half)] for half in range(2)]),
     "hidden_late": ("keep", [P, WOVEN // 2], BF16, rotate([("hidden", THIRD, 0), ("hidden", THIRD, 1), ("hidden", LAST, 0),
                                                            ("hidden", LAST_A, 1)], 3)),
@@ -125,7 +126,6 @@ def tile_rssm_pa_kernel(tc, prev_state, prev_action, obs_bytes, obs_scale, eps,
         b2_rows = keep.tile([P, 2 * L], BF16)
         eps_sb = keep.tile([P, NT, L], BF16)
         ident = keep.tile([P, P], F32)
-        ident_bf = keep.tile([P, P], BF16)
 
         tile_of, before = {}, {}
         for family, (pool_name, shape, dtype, lists) in BUFFERS.items():
@@ -237,18 +237,6 @@ def tile_rssm_pa_kernel(tc, prev_state, prev_action, obs_bytes, obs_scale, eps,
             else:
                 copy[engine](out=woven.rearrange("p (s r e t) -> p r t e s", r=RUNS, e=2, t=4)[:, r0:r1],
                              in_=raw.rearrange("p t (r e s) -> p r t e s", e=2, s=4)[:, r0:r1])
-
-        def pass_w1(half, g, k):
-            bank = tile_of["pass", half, g, k][:].bitcast(BF16).rearrange("p (c u e) -> p c u e", u=2, e=2)
-            cols = tile_of["raw", half, g][:, :, QT * k:QT * (k + 1)]
-            for u in range(2):
-                nc.tensor.matmul(bank[:, :, u, :], ident_bf[:], cols[:, 2 * u:2 * u + 2, :].rearrange("p e c -> p c e"),
-                                 start=True, stop=True)
-
-        def drain_w1(half, g, k):
-            m0 = QT * k // 4
-            out = tile_of["w", half, g][:].bitcast(F32).rearrange("p (s m v) -> p m s v", s=4, v=2)[:, m0:m0 + QT // 4]
-            nc.scalar.copy(out=out, in_=tile_of["pass", half, g, k][:].rearrange("p (m s v) -> p m s v", s=4, v=2))
 
         def quant_w1(half, g):
             cols = slice(KP * half, KP * half + KP)
@@ -407,7 +395,6 @@ def tile_rssm_pa_kernel(tc, prev_state, prev_action, obs_bytes, obs_scale, eps,
                     load_w1: ([], [("raw",) + a]), load_w2: ([], [("raw2",) + a]), load_state: ([], [("state",) + a]),
                     load_action: ([], [("wide",) + a + (MIXED,), ("rows",) + a + (MIXED,)]),
                     quant_x: ([("x",) + a], [("xq",) + a]),
-                    pass_w1: ([("raw",) + a[:2]], [("pass",) + a]), drain_w1: ([("pass",) + a], [("w",) + a[:2]]),
                     weave_w1: ([("raw",) + a[:2]], [("w",) + a[:2]]), quant_w1: ([("w",) + a], [("wq",) + a]),
                     weave_w2: ([("raw2",) + a[:1]], [("w2",) + a[:2]]), quant_w2: ([("w2",) + a[:2]], [("w2q",) + a[:2]]),
                     quant_h: ([("h",) + a], [("hq",) + a])}[f]
@@ -444,8 +431,8 @@ def tile_rssm_pa_kernel(tc, prev_state, prev_action, obs_bytes, obs_scale, eps,
         sync_q += [w1_loads[6], (load_state, 2), obs[7], (load_action, 3)] + w1_loads[7:] + [(load_w2, 0), (load_w2, 1), (load_state, 3), (load_b2,), (load_eps,)] + stores
 
         ALL = (4, 5, 2, 3, 0, 1)
-        tensor_q = steps(turn, (0, 4), (0, 5), (1, 4), (1, 5)) + steps(pass_w1, (0, 5, 0), (0, 5, 1)) + steps(turn, (0, 2), (0, 3)) + [(mm1, FRONT, 0, SL, (4,))]
-        tensor_q += steps(turn, (1, 2), (1, 3)) + [(mm1, FRONT, 0, SL, (5,))] + steps(turn, (0, 0), (0, 1)) + [(mm1, FRONT, 0, (0, 1), (2,))]
+        tensor_q = steps(turn, (0, 4), (0, 5), (1, 4), (1, 5), (0, 2), (1, 2)) + [(mm1, FRONT, 0, SL, (4,))]
+        tensor_q += steps(turn, (0, 3), (1, 3)) + [(mm1, FRONT, 0, SL, (5,))] + steps(turn, (0, 0), (0, 1)) + [(mm1, FRONT, 0, (0, 1), (2,))]
         tensor_q += steps(turn, (1, 0), (1, 1)) + [(mm1, FRONT, 0, (2, 3), (2,))] + steps(turn, (2, 4), (2, 5)) + [(mm1, FRONT, 0, SL, (3,))]
         tensor_q += steps(turn, (2, 2), (2, 3)) + [(mm1, FRONT, 0, SL, (0,))]
         tensor_q += steps(turn, (2, 0), (2, 1)) + [(mm1, FRONT, 0, SL, (1,))] + steps(turn, (3, 4), (3, 5))
@@ -455,23 +442,23 @@ def tile_rssm_pa_kernel(tc, prev_state, prev_action, obs_bytes, obs_scale, eps,
         tensor_q += [(mm1, LAST, 0, (2, 3), ALL), (heads, 3, (0, 1)), (heads, 4, (0, 1)), (mm1, LAST_A, 1, SL, ALL), (heads, 5, (0, 1))]
         tensor_q += [(mm1, LAST_B, 1, SL, ALL), (heads, 6, (0, 1)), (heads, 7, (0,)), (heads, 7, (1,))]
 
-        gpsimd_q = [by("gpsimd", 0, 4, 0, 32), by("gpsimd", 0, 2, 0, 56), by("gpsimd", 0, 3, 0, 56)]
+        gpsimd_q = [by("gpsimd", 0, 4, 0, 32), by("gpsimd", 0, 5, 0, 40), by("gpsimd", 0, 2, 0, 56), by("gpsimd", 0, 3, 0, 56)]
         gpsimd_q += [by("gpsimd", 0, 1, 0, 54), by("gpsimd", 1, 5, 0, 56), (weave_w2, 0, 0, KP, "gpsimd", 0, 64), (weave_w2, 0, KP, SPLIT, "gpsimd", 0, 32), (weave_w2, 1, KP, SPLIT, "gpsimd", 0, 20)]
         gpsimd_q += [(weave_h, THIRD, 0, "gpsimd")]
 
-        scalar_q = [(widen, 1, LATE, 1, "scalar"), (widen, 0, LATE + 1, 1, "scalar"), (widen, 1, LATE + 1, 1, "scalar")] + widens(1, LATE) + [by("scalar", 0, 4, 32)]
-        scalar_q += widens(0, MIXED) + steps(drain_w1, (0, 5, 0), (0, 5, 1)) + widens(1, MIXED) + [by("scalar", 0, 2, 56), by("scalar", 0, 0), by("scalar", 0, 3, 56)] + steps(drain, (0, 0), (0, 1)) + widens(2, LATE) + steps(drain, (1, 0), (1, 1))
+        scalar_q = [(widen, 1, LATE, 1, "scalar"), (widen, 0, LATE + 1, 1, "scalar"), (widen, 1, LATE + 1, 1, "scalar")] + widens(1, LATE) + [by("scalar", 0, 4, 32), by("scalar", 0, 5, 40)]
+        scalar_q += widens(0, MIXED) + widens(1, MIXED) + [by("scalar", 0, 2, 56), by("scalar", 0, 0), by("scalar", 0, 3, 56)] + steps(drain, (0, 0), (0, 1)) + widens(2, LATE) + steps(drain, (1, 0), (1, 1))
         scalar_q += widens(2, MIXED) + [by("scalar", 0, 1, 54), by("scalar", 1, 4)] + widens(3, LATE) + steps(drain, (2, 0), (2, 1)) + [by("scalar", 1, 5, 56)] + relus(FRONT, 0)
         scalar_q += [by("scalar", 1, 2), by("scalar", 1, 3, 20)] + relus(THIRD, 0, (0, 1)) + widens(3, MIXED) + relus(THIRD, 0, (2, 3)) + [(weave_w2, 1, 0, KP, "scalar", 0, 64), (weave_h, FRONT_A, 0, "scalar")]
         scalar_q += relus(FRONT, 1) + [(weave_h, FRONT_A, 1, "scalar")] + steps(drain, (3, 0), (3, 1)) + [(weave_h, FRONT_B, 0, "scalar"), (weave_h, FRONT_B, 1, "scalar")]
 
         vector_q = [(widen, 0, LATE, 1, "vector")] + steps(product, (0, 4), (0, 5), (1, 4), (1, 5))
         vector_q += [(quant_w1, 0, 4), (quant_x, 0, 4), (quant_w1, 0, 5), (quant_x, 0, 5)] + steps(product, (0, 2), (1, 2))
-        vector_q += [(quant_w1, 0, 2), (quant_x, 0, 2)] + steps(product, (0, 3), (1, 3)) + [(quant_w1, 0, 3), (quant_x, 0, 3), (quant_w1, 0, 0), (quant_x, 0, 0)]
+        vector_q += [(quant_w1, 0, 2), (quant_x, 0, 2)] + steps(product, (0, 3), (1, 3)) + [(quant_w1, 0, 3), (quant_x, 0, 3), (quant_x, 0, 0), (quant_w1, 0, 0)]
         vector_q += steps(product, (2, 4), (2, 5)) + [(quant_x, 0, 1), (quant_w1, 0, 1), (quant_w1, 1, 4), (quant_x, 1, 4)] + steps(product, (2, 2), (2, 3))
         vector_q += [(quant_w1, 1, 5), (quant_x, 1, 2), (quant_x, 1, 0), by("vector", 1, 0), (quant_w1, 1, 2), (quant_w1, 1, 0), by("vector", 1, 3, 0, 20), by("vector", 1, 1), (quant_w1, 1, 3), (quant_w1, 1, 1)]
         vector_q += steps(product, (3, 4), (3, 5), (3, 2), (3, 3))
-        vector_q += [(quant_w2, 0, 0, KP), (quant_w2, 1, 0, KP), (weave_w2, 1, KP, SPLIT, "vector", 20, 32), (quant_w2, 0, KP, SPLIT), (quant_h, FRONT_A, 0), (quant_w2, 1, KP, SPLIT), (quant_x, 2, 4), (quant_h, FRONT_A, 1), (quant_x, 2, 2), (quant_x, 2, 0)]
+        vector_q += [(quant_w2, 0, 0, KP), (quant_w2, 1, 0, KP), (weave_w2, 1, KP, SPLIT, "vector", 20, 32), (quant_w2, 0, KP, SPLIT), (quant_h, FRONT_A, 0), (quant_w2, 1, KP, SPLIT), (quant_x, 2, 4), (quant_h, FRONT_A, 1), (quant_x, 2, 0), (quant_x, 2, 2)]
 
         def sample(n):
             return [(noise, n, 1, 0, L), (shift, n, 1, 0, L, "vector")]
@@ -498,7 +485,6 @@ def tile_rssm_pa_kernel(tc, prev_state, prev_action, obs_bytes, obs_scale, eps,
 
         nc.vector.memset(ones[:], 1.0)
         make_identity(nc, ident[:])
-        make_identity(nc, ident_bf[:])
         nc.scalar.activation(scale_mixed[:ACTION_ROWS, :], ones[:], ACT.Sqrt)
 
         queues = [sync_q, tensor_q, scalar_q, vector_q, gpsimd_q]

@@ -220,8 +220,8 @@ def tile_rssm_pa_kernel(tc, prev_state, prev_action, obs_bytes, obs_scale, eps,
         def product(q, g):
             scale = scale_mixed[:] if g == MIXED else scale_obs[:, g - MIXED - 1, :]
             nc.vector.tensor_tensor(out=x_half(q, g).rearrange("p (r u e) -> p r u e", u=2, e=2),
-                                    in0=tile_of["turn", q, g][:].bitcast(BF16).rearrange("p (u r e) -> p r u e", u=2, e=2),
-                                    in1=scale.rearrange("p (u e) -> p u e", e=2).unsqueeze(1).to_broadcast([P, QT, 2, 2]),
+                                    in1=tile_of["turn", q, g][:].bitcast(BF16).rearrange("p (u r e) -> p r u e", u=2, e=2),
+                                    in0=scale.rearrange("p (u e) -> p u e", e=2).unsqueeze(1).to_broadcast([P, QT, 2, 2]),
                                     op=ALU.mult)
 
         def quant_x(grp, g):

@@ -35,7 +35,7 @@ THIRD, LAST, LAST_A, LAST_B = (1, 0, QT), (2, 0, QT), (2, 0, P), (2, P, P)
 W2_PIECES = tuple((g, c0, min(KP, 2 * L - c0)) for g in range(G2) for c0 in (0, KP))
 H_PIECES = ((FRONT_A, 0), (FRONT_B, 0), (FRONT_A, 1), (FRONT_B, 1), (THIRD, 0), (THIRD, 1), (LAST, 0), (LAST_A, 1), (LAST_B, 1))
 CUT = 2 * KP - A
-OBS_LOADS = ((0, 1, CUT, CUT + KP), (1, 1, CUT, CUT + KP), (0, 2, CUT + KP, O), (2, 2, CUT, O), (0, 2, 0, CUT), (2, 2, 0, CUT), (4, 2, 0, O), (6, 2, 0, O))
+OBS_LOADS = ((0, 1, CUT, CUT + KP), (1, 1, CUT, CUT + KP), (2, 2, CUT, CUT + KP), (0, 4, CUT + KP, O), (0, 2, 0, CUT), (2, 2, 0, CUT), (4, 2, 0, O), (6, 2, 0, O))
 
 
 def rotate(keys, depth):
@@ -54,13 +54,13 @@ W1_LOADS = [(0, 4), (0, 5), (0, 2), (0, 0), (0, 3), (0, 1), (1, 4), (1, 5), (1, 
 HEADS = rotate([("head", n, c0) for n in range(NT) for c0 in (SPLIT, 0)], 4)
 BANKS = [
     turned((0, 4), (0, 2), (0, 0), (1, 0), (2, 2)) + [("acc", THIRD, 0, 0)] + turned((3, 2)) + [("acc", THIRD, 1, 0), ("acc", LAST, 0, 2), ("acc", LAST_B, 1, 1)],
-    turned((0, 5), (1, 2), (0, 1), (1, 1), (2, 3)) + [("acc", THIRD, 0, 2)] + turned((3, 3)) + [("acc", THIRD, 1, 2), ("acc", LAST_B, 1, 2)],
-    turned((1, 4), (0, 3), (2, 4), (2, 0), (3, 4), (3, 0)) + [("acc", LAST, 0, 0), ("acc", LAST_B, 1, 0)],
+    turned((1, 4), (1, 2), (0, 1), (1, 1), (2, 3)) + [("acc", THIRD, 0, 2)] + turned((3, 3)) + [("acc", THIRD, 1, 2), ("acc", LAST_B, 1, 2)],
+    turned((0, 5), (0, 3), (2, 4), (2, 0), (3, 4), (3, 0)) + [("acc", LAST, 0, 0), ("acc", LAST_B, 1, 0)],
     turned((1, 5), (1, 3), (2, 5), (2, 1), (3, 5), (3, 1)) + [("acc", LAST_A, 1, 0), ("acc", LAST_B, 1, 3)],
 ] + [[("acc", FRONT, 0, t), ("acc", FRONT, 1, t)] + HEADS[t] for t in range(4)]
 WOVEN_LISTS = [
-    w((0, 5), (0, 2), (0, 3), (1, 4), (1, 5), (1, 3)) + [("w2", 0, 0)],
-    w((0, 4), (0, 0), (1, 0)) + [("w2", 1, 0)],
+    w((0, 4), (0, 5), (0, 2), (0, 3), (1, 4), (1, 5), (1, 3)) + [("w2", 0, 0)],
+    w((0, 0), (1, 0)) + [("w2", 1, 0)],
     [("x", 0, 0)] + w((0, 1), (1, 2)) + [("x", 2, 2)],
     w((1, 1)) + [("w2", 1, KP)],
     [("x", 0, 4), ("x", 0, 3), ("x", 1, 2), ("x", 2, 4)],
@@ -72,12 +72,12 @@ NARROW_LISTS = rotate([("w2", 0, KP), ("h", FRONT_A, 0), ("h", FRONT_A, 1), ("h"
                        ("h", THIRD, 1), ("h", LAST, 0), ("h", LAST_A, 1), ("h", LAST_B, 1)], 4)
 SLICES_A_BANK = {FRONT: 1, THIRD: 2, LAST: 2, LAST_A: 4, LAST_B: 1}
 PIECE = 64
-POOL_COLS = 5 * PIECE
+G0, GE, GR, GW, VR = 32, 44, 50, 8, 20
 BUFFERS = {
     "bank": ("psum", [P, KP], F32, BANKS),
     "obs": ("keep", [P, 2 * O], U8, [[("obs", 0, CUT), ("obs", 4, 0)], [("obs", 1, CUT), ("obs", 6, 0)]]),
-    "obs_second": ("keep", [P, 2 * KP], U8, [[("obs", 0, CUT + KP)]]),
-    "obs_front": ("keep", [P, 4 * KP], U8, [[("obs", 2, CUT)], [("obs", 0, 0)], [("obs", 2, 0)]]),
+    "obs_second": ("keep", [P, 2 * KP], U8, [[("obs", 2, CUT)]]),
+    "obs_front": ("keep", [P, 4 * KP], U8, [[("obs", 0, CUT + KP)], [("obs", 0, 0)], [("obs", 2, 0)]]),
     "wide": ("keep", [P, 4 * KP], BF16, [[("wide", q, g), ("wide", q + 2, g)] for q in range(2) for g in (MIXED, LATE)]),
     "state": ("keep", [P, 2, S], BF16, rotate([("state", q) for q in range(4)], 2)),
     "raw": ("keep", [P, 4, KP], BF16, rotate([("raw",) + key for key in W1_LOADS], 6)),
@@ -292,11 +292,11 @@ def tile_rssm_pa_kernel(tc, prev_state, prev_action, obs_bytes, obs_scale, eps,
         def parent(span):
             return FRONT if span[0] == 0 else span
 
-        def weave_h(span, half, engine):
+        def weave_h(span, half, engine, n0=0, n1=None):
             whole = parent(span)
             src = tile_of["hidden", whole, half][:, :4 * whole[2]].rearrange("p (t n) -> p t n", t=4)
-            r0 = span[1] - whole[1]
-            weave(tile_of["h", span, half][:, :4 * span[2]], src[:, :, r0:r0 + span[2]], engine)
+            r0, n1 = span[1] - whole[1], n1 or span[2]
+            weave(tile_of["h", span, half][:, 4 * n0:4 * n1], src[:, :, r0 + n0:r0 + n1], engine)
 
         def quant_h(span, half):
             grp, r0, n = span
@@ -422,43 +422,44 @@ def tile_rssm_pa_kernel(tc, prev_state, prev_action, obs_bytes, obs_scale, eps,
         obs = [(load_obs,) + a for a in OBS_LOADS]
         w1_loads = [(load_w1,) + key for key in W1_LOADS]
         stores = []
-        for n in range(NT):
-            earlier = [(store_sample, n - 1, 1, 0, L)] if n else []
-            stores += [(store_std, n)] + (earlier + [(store_mean, n)] if n >= NT - 2 else [(store_mean, n)] + earlier)
+        for n in range(NT - 2):
+            stores += [(store_std, n), (store_mean, n)] + [(store_sample, n - 3, 2, 0, L)] * (n in (3, 5))
+        stores += [(store_sample, 4, 1, 0, L), (store_std, 6), (store_sample, 5, 1, 0, L), (store_mean, 6), (store_std, 7), (store_mean, 7), (store_sample, 6, 1, 0, L)]
         stores += steps(store_sample, (NT - 1, 1, 0, L // 2), (NT - 1, 1, L // 2, L))
-        sync_q = obs[:2] + [(load_scales,)] + obs[2:4] + w1_loads[:2] + [obs[4], (load_action, 0), obs[5], (load_action, 1), (load_mixed_scales,)]
-        sync_q += w1_loads[2:5] + [(load_state, 0), (load_state, 1), obs[6], (load_action, 2), w1_loads[5], (load_b1,)]
+        sync_q = obs[:2] + [(load_scales,), obs[2], w1_loads[0], obs[3], w1_loads[1], obs[4], (load_action, 0), obs[5], (load_action, 1), (load_mixed_scales,)]
+        sync_q += w1_loads[2:4] + [(load_state, 0), w1_loads[4], (load_state, 1), obs[6], (load_action, 2), w1_loads[5], (load_b1,)]
         sync_q += [w1_loads[6], (load_state, 2), obs[7], (load_action, 3)] + w1_loads[7:] + [(load_w2, 0), (load_w2, 1), (load_state, 3), (load_b2,), (load_eps,)] + stores
 
         ALL = (4, 5, 2, 3, 0, 1)
-        tensor_q = steps(turn, (0, 4), (0, 5), (1, 4), (1, 5), (0, 2), (1, 2)) + [(mm1, FRONT, 0, SL, (4,))]
-        tensor_q += steps(turn, (0, 3), (1, 3)) + [(mm1, FRONT, 0, SL, (5,))] + steps(turn, (0, 0), (0, 1)) + [(mm1, FRONT, 0, (0, 1), (2,))]
+        tensor_q = steps(turn, (0, 4), (1, 4), (0, 5), (1, 5)) + [(mm1, FRONT, 0, (0, 1, 2), (4,))] + steps(turn, (0, 2), (1, 2)) + [(mm1, FRONT, 0, (3,), (4,)), (mm1, FRONT, 0, (0, 1), (5,))]
+        tensor_q += steps(turn, (0, 3), (0, 0)) + [(mm1, FRONT, 0, (2, 3), (5,))] + steps(turn, (1, 3), (0, 1)) + [(mm1, FRONT, 0, (0, 1), (2,))]
         tensor_q += steps(turn, (1, 0), (1, 1)) + [(mm1, FRONT, 0, (2, 3), (2,))] + steps(turn, (2, 4), (2, 5)) + [(mm1, FRONT, 0, SL, (3,))]
         tensor_q += steps(turn, (2, 2), (2, 3)) + [(mm1, FRONT, 0, SL, (0,))]
         tensor_q += steps(turn, (2, 0), (2, 1)) + [(mm1, FRONT, 0, SL, (1,))] + steps(turn, (3, 4), (3, 5))
-        tensor_q += [(mm1, THIRD, 0, (0, 1), ALL[:2]), (mm1, FRONT, 1, SL, (4, 5)), (mm1, THIRD, 0, (0, 1), ALL[2:]), (mm1, THIRD, 0, (2, 3), ALL), (mm1, FRONT, 1, SL, (2, 0))]
+        tensor_q += [(mm1, THIRD, 0, (0, 1), ALL[:2]), (mm1, FRONT, 1, SL, (4, 5)), (mm1, THIRD, 0, (0, 1), ALL[2:]), (mm1, THIRD, 0, (2, 3), ALL), (mm1, FRONT, 1, SL, (0, 2))]
         tensor_q += steps(turn, (3, 2), (3, 3)) + [(mm1, FRONT, 1, SL, (3, 1))] + steps(turn, (3, 0), (3, 1))
-        tensor_q += [(mm1, THIRD, 1, SL, ALL), (heads, 0, (0, 1)), (heads, 1, (0, 1)), (mm1, LAST, 0, (0, 1), ALL), (heads, 2, (0, 1))]
-        tensor_q += [(mm1, LAST, 0, (2, 3), ALL), (heads, 3, (0, 1)), (heads, 4, (0, 1)), (mm1, LAST_A, 1, SL, ALL), (heads, 5, (0, 1))]
+        tensor_q += [(mm1, THIRD, 1, SL, ALL), (heads, 0, (0, 1)), (heads, 1, (0, 1)), (mm1, LAST, 0, (0, 1), (4, 5, 0, 1, 2, 3))]
+        tensor_q += [(mm1, LAST, 0, (2, 3), ALL), (heads, 2, (0, 1)), (heads, 3, (0, 1)), (mm1, LAST_A, 1, SL, ALL), (heads, 4, (0, 1)), (heads, 5, (0, 1))]
         tensor_q += [(mm1, LAST_B, 1, SL, ALL), (heads, 6, (0, 1)), (heads, 7, (0,)), (heads, 7, (1,))]
 
-        gpsimd_q = [by("gpsimd", 0, 4, 0, 32), by("gpsimd", 0, 5, 0, 40), by("gpsimd", 0, 2, 0, 56), by("gpsimd", 0, 3, 0, 56)]
-        gpsimd_q += [by("gpsimd", 0, 1, 0, 54), by("gpsimd", 1, 5, 0, 56), (weave_w2, 0, 0, KP, "gpsimd", 0, 64), (weave_w2, 0, KP, SPLIT, "gpsimd", 0, 32), (weave_w2, 1, KP, SPLIT, "gpsimd", 0, 20)]
-        gpsimd_q += [(weave_h, THIRD, 0, "gpsimd")]
+        gpsimd_q = [by("gpsimd", 0, 4, 0, G0)] + [by("gpsimd", 0, g, 0, GE) for g in (5, 2)] + [by("gpsimd", 0, 3, 0, GR)]
+        gpsimd_q += [by("gpsimd", 0, 1, 0, GR), by("gpsimd", 1, 5, 0, GR), (weave_w2, 0, 0, KP, "gpsimd", 0, 64), (weave_w2, 0, KP, SPLIT, "gpsimd", 0, 32), (weave_w2, 1, KP, SPLIT, "gpsimd", 0, GW)]
+        gpsimd_q += [(weave_h, THIRD, 0, "gpsimd"), (shift, 1, 1, 0, L, "gpsimd"), (shift, 3, 1, 0, L, "gpsimd")]
 
-        scalar_q = [(widen, 1, LATE, 1, "scalar"), (widen, 0, LATE + 1, 1, "scalar"), (widen, 1, LATE + 1, 1, "scalar")] + widens(1, LATE) + [by("scalar", 0, 4, 32), by("scalar", 0, 5, 40)]
-        scalar_q += widens(0, MIXED) + widens(1, MIXED) + [by("scalar", 0, 2, 56), by("scalar", 0, 0), by("scalar", 0, 3, 56)] + steps(drain, (0, 0), (0, 1)) + widens(2, LATE) + steps(drain, (1, 0), (1, 1))
-        scalar_q += widens(2, MIXED) + [by("scalar", 0, 1, 54), by("scalar", 1, 4)] + widens(3, LATE) + steps(drain, (2, 0), (2, 1)) + [by("scalar", 1, 5, 56)] + relus(FRONT, 0)
-        scalar_q += [by("scalar", 1, 2), by("scalar", 1, 3, 20)] + relus(THIRD, 0, (0, 1)) + widens(3, MIXED) + relus(THIRD, 0, (2, 3)) + [(weave_w2, 1, 0, KP, "scalar", 0, 64), (weave_h, FRONT_A, 0, "scalar")]
-        scalar_q += relus(FRONT, 1) + [(weave_h, FRONT_A, 1, "scalar")] + steps(drain, (3, 0), (3, 1)) + [(weave_h, FRONT_B, 0, "scalar"), (weave_h, FRONT_B, 1, "scalar")]
+        scalar_q = [(widen, n, LATE, 1, "scalar") for n in (1, 2, 3)] + [by("scalar", 0, 4, G0)] + [(widen, n, LATE + 1, 1, "scalar") for n in range(4)]
+        scalar_q += [(widen, n, MIXED, 1, "scalar") for n in range(4)] + [by("scalar", 0, 5, GE)] + [(widen, n, MIXED + 1, 1, "scalar") for n in range(4)]
+        scalar_q += [by("scalar", 0, 2, GE), by("scalar", 0, 0), (drain, 0, 0), by("scalar", 0, 3, GR), (drain, 0, 1)] + widens(2, LATE) + steps(drain, (1, 0), (1, 1))
+        scalar_q += widens(2, MIXED) + [by("scalar", 0, 1, GR), by("scalar", 1, 4)] + widens(3, LATE) + steps(drain, (2, 0), (2, 1)) + [by("scalar", 1, 5, GR)] + relus(FRONT, 0)
+        scalar_q += [by("scalar", 1, 2), by("scalar", 1, 3, VR)] + relus(THIRD, 0, (0, 1)) + widens(3, MIXED) + relus(THIRD, 0, (2, 3)) + [(weave_w2, 1, 0, KP, "scalar", 0, 64), (weave_h, FRONT_A, 0, "scalar")]
+        scalar_q += relus(FRONT, 1) + [(drain, 3, 0), (weave_h, FRONT_A, 1, "scalar"), (drain, 3, 1), (weave_h, FRONT_B, 0, "scalar")] + relus(THIRD, 1, (0, 1)) + [(weave_h, FRONT_B, 1, "scalar")]
 
-        vector_q = [(widen, 0, LATE, 1, "vector")] + steps(product, (0, 4), (0, 5), (1, 4), (1, 5))
-        vector_q += [(quant_w1, 0, 4), (quant_x, 0, 4), (quant_w1, 0, 5), (quant_x, 0, 5)] + steps(product, (0, 2), (1, 2))
+        vector_q = [(widen, 0, LATE, 1, "vector")] + steps(product, (0, 4), (1, 4)) + [(quant_w1, 0, 4), (quant_x, 0, 4)]
+        vector_q += steps(product, (0, 5), (1, 5)) + [(quant_w1, 0, 5), (quant_x, 0, 5)] + steps(product, (0, 2), (1, 2))
         vector_q += [(quant_w1, 0, 2), (quant_x, 0, 2)] + steps(product, (0, 3), (1, 3)) + [(quant_w1, 0, 3), (quant_x, 0, 3), (quant_x, 0, 0), (quant_w1, 0, 0)]
         vector_q += steps(product, (2, 4), (2, 5)) + [(quant_x, 0, 1), (quant_w1, 0, 1), (quant_w1, 1, 4), (quant_x, 1, 4)] + steps(product, (2, 2), (2, 3))
-        vector_q += [(quant_w1, 1, 5), (quant_x, 1, 2), (quant_x, 1, 0), by("vector", 1, 0), (quant_w1, 1, 2), (quant_w1, 1, 0), by("vector", 1, 3, 0, 20), by("vector", 1, 1), (quant_w1, 1, 3), (quant_w1, 1, 1)]
+        vector_q += [(quant_w1, 1, 5), (quant_x, 1, 2), (quant_x, 1, 0), by("vector", 1, 0), by("vector", 1, 3, 0, VR), (quant_w1, 1, 0), (quant_w1, 1, 2), by("vector", 1, 1), (quant_w1, 1, 3), (quant_w1, 1, 1)]
         vector_q += steps(product, (3, 4), (3, 5), (3, 2), (3, 3))
-        vector_q += [(quant_w2, 0, 0, KP), (quant_w2, 1, 0, KP), (weave_w2, 1, KP, SPLIT, "vector", 20, 32), (quant_w2, 0, KP, SPLIT), (quant_h, FRONT_A, 0), (quant_w2, 1, KP, SPLIT), (quant_x, 2, 4), (quant_h, FRONT_A, 1), (quant_x, 2, 0), (quant_x, 2, 2)]
+        vector_q += [(quant_w2, 0, 0, KP), (quant_w2, 1, 0, KP), (weave_w2, 1, KP, SPLIT, "vector", GW, 32), (quant_w2, 0, KP, SPLIT), (quant_h, FRONT_A, 0), (quant_w2, 1, KP, SPLIT), (quant_h, FRONT_A, 1), (quant_x, 2, 4), (quant_x, 2, 0), (quant_x, 2, 2)]
 
         def sample(n):
             return [(noise, n, 1, 0, L), (shift, n, 1, 0, L, "vector")]
@@ -467,14 +468,13 @@ def tile_rssm_pa_kernel(tc, prev_state, prev_action, obs_bytes, obs_scale, eps,
             return (root, n, 0, L)
 
         end, mid = NT - 1, L // 2
-        scalar_q += [rooted(0)] + relus(THIRD, 1, (0, 1)) + [rooted(1)] + relus(THIRD, 1, (2, 3)) + relus(LAST, 0, (0, 1)) + [(weave_h, THIRD, 1, "scalar"), rooted(2)] + relus(LAST, 0, (2, 3))
-        scalar_q += [rooted(3), (weave_h, LAST, 0, "scalar"), rooted(4)] + relus(LAST_A, 1) + [(weave_h, LAST_A, 1, "scalar"), (relu_woven, LAST_B, 1, 0, "scalar"), rooted(5)] + [(relu_woven, LAST_B, 1, t, "scalar") for t in SL[1:]] + [rooted(6), (root, end, 0, mid), (root, end, mid, L)]
-        vector_q += [wide(0), wide(1), narrow(0), narrow(1), (quant_h, FRONT_B, 0), (quant_h, FRONT_B, 1), sample(0)[0], (quant_h, THIRD, 0), sample(0)[1]]
-        vector_q += [sample(1)[0], wide(2), sample(1)[1], narrow(2), (quant_h, THIRD, 1)]
-        for n in (3, 4):
-            vector_q += [wide(n), sample(n - 1)[0], narrow(n), sample(n - 1)[1]]
-        vector_q += [(quant_h, LAST, 0), wide(5), sample(4)[0], narrow(5), (quant_h, LAST_A, 1), sample(4)[1], sample(5)[0], wide(6), sample(5)[1], (quant_h, LAST_B, 1), narrow(6)]
-        vector_q += [sample(6)[0], (bias, end, L, L + mid), (bias, end, L + mid, 2 * L), sample(6)[1], narrow(end), (bias, end, SPLIT, L)]
+        scalar_q += [rooted(0)] + relus(THIRD, 1, (2, 3)) + [rooted(1), (weave_h, THIRD, 1, "scalar")] + relus(LAST, 0) + [rooted(2)]
+        scalar_q += [(weave_h, LAST, 0, "scalar", 0, P), rooted(3), (weave_h, LAST, 0, "scalar", P)] + relus(LAST_A, 1) + [(weave_h, LAST_A, 1, "scalar"), rooted(4)]
+        scalar_q += [(relu_woven, LAST_B, 1, t, "scalar") for t in SL[:1]] + [rooted(5)] + [(relu_woven, LAST_B, 1, t, "scalar") for t in SL[1:]] + [rooted(6), (root, end, 0, mid), (root, end, mid, L)]
+        vector_q += [wide(0), wide(1), narrow(0), narrow(1), (quant_h, FRONT_B, 0), (quant_h, FRONT_B, 1), sample(0)[0], (quant_h, THIRD, 0), sample(1)[0], sample(0)[1]]
+        vector_q += [wide(2), narrow(2), wide(3), narrow(3), (quant_h, THIRD, 1), sample(2)[0], sample(3)[0], sample(2)[1], wide(4), narrow(4), wide(5), narrow(5)]
+        vector_q += [(quant_h, LAST, 0), (quant_h, LAST_A, 1), sample(4)[0], sample(5)[0], sample(4)[1], wide(6), (quant_h, LAST_B, 1), sample(5)[1], narrow(6)]
+        vector_q += [(bias, end, L, L + mid), (bias, end, L + mid, 2 * L), sample(6)[0], narrow(end), (bias, end, SPLIT, L), sample(6)[1]]
         vector_q += [(noise, end, 1, 0, mid), (noise, end, 1, mid, L), (shift, end, 1, 0, mid, "vector"), (shift, end, 1, mid, L, "vector")]
 
         in_bank = {}

@@ -72,7 +72,7 @@ NARROW_LISTS = rotate([("w2", 0, KP), ("h", FRONT_A, 0), ("h", FRONT_A, 1), ("h"
                        ("h", THIRD, 1), ("h", LAST, 0), ("h", LAST_A, 1), ("h", LAST_B, 1)], 4)
 SLICES_A_BANK = {FRONT: 1, THIRD: 2, LAST: 2, LAST_A: 4, LAST_B: 1}
 PIECE = 64
-G0, GE, GR, GW, VR = 32, 44, 50, 8, 20
+G0, GE, GR, VR = 32, 44, 48, 20
 BUFFERS = {
     "bank": ("psum", [P, KP], F32, BANKS),
     "obs": ("keep", [P, 2 * O], U8, [[("obs", 0, CUT), ("obs", 4, 0)], [("obs", 1, CUT), ("obs", 6, 0)]]),
@@ -443,8 +443,8 @@ def tile_rssm_pa_kernel(tc, prev_state, prev_action, obs_bytes, obs_scale, eps,
         tensor_q += [(mm1, LAST_B, 1, SL, ALL), (heads, 6, (0, 1)), (heads, 7, (0,)), (heads, 7, (1,))]
 
         gpsimd_q = [by("gpsimd", 0, 4, 0, G0)] + [by("gpsimd", 0, g, 0, GE) for g in (5, 2)] + [by("gpsimd", 0, 3, 0, GR)]
-        gpsimd_q += [by("gpsimd", 0, 1, 0, GR), by("gpsimd", 1, 5, 0, GR), (weave_w2, 0, 0, KP, "gpsimd", 0, 64), (weave_w2, 0, KP, SPLIT, "gpsimd", 0, 32), (weave_w2, 1, KP, SPLIT, "gpsimd", 0, GW)]
-        gpsimd_q += [(weave_h, THIRD, 0, "gpsimd"), (shift, 1, 1, 0, L, "gpsimd"), (shift, 3, 1, 0, L, "gpsimd")]
+        gpsimd_q += [by("gpsimd", 0, 1, 0, GR), by("gpsimd", 1, 5, 0, GR), (weave_w2, 0, 0, KP, "gpsimd", 0, 64), (weave_w2, 0, KP, SPLIT, "gpsimd", 0, 32)]
+        gpsimd_q += [(weave_h, THIRD, 0, "gpsimd")]
 
         scalar_q = [(widen, n, LATE, 1, "scalar") for n in (1, 2, 3)] + [by("scalar", 0, 4, G0)] + [(widen, n, LATE + 1, 1, "scalar") for n in range(4)]
         scalar_q += [(widen, n, MIXED, 1, "scalar") for n in range(4)] + [by("scalar", 0, 5, GE)] + [(widen, n, MIXED + 1, 1, "scalar") for n in range(4)]
@@ -459,7 +459,7 @@ def tile_rssm_pa_kernel(tc, prev_state, prev_action, obs_bytes, obs_scale, eps,
         vector_q += steps(product, (2, 4), (2, 5)) + [(quant_x, 0, 1), (quant_w1, 0, 1), (quant_w1, 1, 4), (quant_x, 1, 4)] + steps(product, (2, 2), (2, 3))
         vector_q += [(quant_w1, 1, 5), (quant_x, 1, 2), (quant_x, 1, 0), by("vector", 1, 0), by("vector", 1, 3, 0, VR), (quant_w1, 1, 0), (quant_w1, 1, 2), by("vector", 1, 1), (quant_w1, 1, 3), (quant_w1, 1, 1)]
         vector_q += steps(product, (3, 4), (3, 5), (3, 2), (3, 3))
-        vector_q += [(quant_w2, 0, 0, KP), (quant_w2, 1, 0, KP), (weave_w2, 1, KP, SPLIT, "vector", GW, 32), (quant_w2, 0, KP, SPLIT), (quant_h, FRONT_A, 0), (quant_w2, 1, KP, SPLIT), (quant_h, FRONT_A, 1), (quant_x, 2, 4), (quant_x, 2, 0), (quant_x, 2, 2)]
+        vector_q += [(quant_w2, 0, 0, KP), (quant_w2, 1, 0, KP), (weave_w2, 1, KP, SPLIT, "vector", 0, 32), (quant_w2, 0, KP, SPLIT), (quant_h, FRONT_A, 0), (quant_w2, 1, KP, SPLIT), (quant_h, FRONT_A, 1), (quant_x, 2, 4), (quant_x, 2, 0), (quant_x, 2, 2)]
 
         def sample(n):
             return [(noise, n, 1, 0, L), (shift, n, 1, 0, L, "vector")]
@@ -471,8 +471,8 @@ def tile_rssm_pa_kernel(tc, prev_state, prev_action, obs_bytes, obs_scale, eps,
         scalar_q += [rooted(0)] + relus(THIRD, 1, (2, 3)) + [rooted(1), (weave_h, THIRD, 1, "scalar")] + relus(LAST, 0) + [rooted(2)]
         scalar_q += [(weave_h, LAST, 0, "scalar", 0, P), rooted(3), (weave_h, LAST, 0, "scalar", P)] + relus(LAST_A, 1) + [(weave_h, LAST_A, 1, "scalar"), rooted(4)]
         scalar_q += [(relu_woven, LAST_B, 1, t, "scalar") for t in SL[:1]] + [rooted(5)] + [(relu_woven, LAST_B, 1, t, "scalar") for t in SL[1:]] + [rooted(6), (root, end, 0, mid), (root, end, mid, L)]
-        vector_q += [wide(0), wide(1), narrow(0), narrow(1), (quant_h, FRONT_B, 0), (quant_h, FRONT_B, 1), sample(0)[0], (quant_h, THIRD, 0), sample(1)[0], sample(0)[1]]
-        vector_q += [wide(2), narrow(2), wide(3), narrow(3), (quant_h, THIRD, 1), sample(2)[0], sample(3)[0], sample(2)[1], wide(4), narrow(4), wide(5), narrow(5)]
+        vector_q += [wide(0), wide(1), narrow(0), narrow(1), (quant_h, FRONT_B, 0), (quant_h, FRONT_B, 1), sample(0)[0], (quant_h, THIRD, 0), sample(1)[0], sample(0)[1], sample(1)[1]]
+        vector_q += [wide(2), narrow(2), wide(3), narrow(3), (quant_h, THIRD, 1), sample(2)[0], sample(3)[0], sample(2)[1], wide(4), sample(3)[1], narrow(4), wide(5), narrow(5)]
         vector_q += [(quant_h, LAST, 0), (quant_h, LAST_A, 1), sample(4)[0], sample(5)[0], sample(4)[1], wide(6), (quant_h, LAST_B, 1), sample(5)[1], narrow(6)]
         vector_q += [(bias, end, L, L + mid), (bias, end, L + mid, 2 * L), sample(6)[0], narrow(end), (bias, end, SPLIT, L), sample(6)[1]]
         vector_q += [(noise, end, 1, 0, mid), (noise, end, 1, mid, L), (shift, end, 1, 0, mid, "vector"), (shift, end, 1, mid, L, "vector")]

@@ -431,11 +431,9 @@ def tile_rssm_pa_kernel(tc, prev_state, prev_action, obs_bytes, obs_scale, eps,
         sync_q += [w1_loads[6], (load_state, 2), obs[7], (load_action, 3)] + w1_loads[7:] + [(load_w2, 0), (load_w2, 1), (load_state, 3), (load_b2,), (load_eps,)] + stores
 
         ALL = (4, 5, 2, 3, 0, 1)
-        tensor_q = steps(turn, (0, 4), (1, 4), (0, 5), (1, 5)) + [(mm1, FRONT, 0, (0, 1, 2), (4,))] + steps(turn, (0, 2), (1, 2)) + [(mm1, FRONT, 0, (3,), (4,)), (mm1, FRONT, 0, (0, 1), (5,))]
-        tensor_q += steps(turn, (0, 3), (0, 0)) + [(mm1, FRONT, 0, (2, 3), (5,))] + steps(turn, (1, 3), (0, 1)) + [(mm1, FRONT, 0, (0, 1), (2,))]
-        tensor_q += steps(turn, (1, 0), (1, 1)) + [(mm1, FRONT, 0, (2, 3), (2,))] + steps(turn, (2, 4), (2, 5)) + [(mm1, FRONT, 0, SL, (3,))]
-        tensor_q += steps(turn, (2, 2), (2, 3)) + [(mm1, FRONT, 0, SL, (0,))]
-        tensor_q += steps(turn, (2, 0), (2, 1)) + [(mm1, FRONT, 0, SL, (1,))] + steps(turn, (3, 4), (3, 5))
+        tensor_q = steps(turn, (0, 4), (1, 4), (0, 5), (1, 5)) + [(mm1, FRONT, 0, SL, (4,))] + steps(turn, (0, 2), (1, 2), (0, 3), (1, 3)) + [(mm1, FRONT, 0, SL, (5,))]
+        tensor_q += steps(turn, (0, 0), (0, 1)) + [(mm1, FRONT, 0, SL, (2,))] + steps(turn, (1, 0), (1, 1), (2, 4), (2, 5)) + [(mm1, FRONT, 0, SL, (3, 0))]
+        tensor_q += steps(turn, (2, 2), (2, 3), (2, 0), (2, 1)) + [(mm1, FRONT, 0, SL, (1,))] + steps(turn, (3, 4), (3, 5))
         tensor_q += [(mm1, THIRD, 0, (0, 1), ALL[:2]), (mm1, FRONT, 1, SL, (4, 5)), (mm1, THIRD, 0, (0, 1), ALL[2:]), (mm1, THIRD, 0, (2, 3), ALL), (mm1, FRONT, 1, SL, (0, 2))]
         tensor_q += steps(turn, (3, 2), (3, 3)) + [(mm1, FRONT, 1, SL, (3, 1))] + steps(turn, (3, 0), (3, 1))
         tensor_q += [(mm1, THIRD, 1, SL, ALL), (heads, 0, (0, 1)), (heads, 1, (0, 1)), (mm1, LAST, 0, (0, 1), (4, 5, 0, 1, 2, 3))]

@@ -50,7 +50,7 @@ def w(*pairs):
     return [("w",) + pair for pair in pairs]
 
 
-W1_LOADS = [(0, 4), (0, 5), (0, 2), (0, 0), (0, 3), (0, 1), (1, 4), (1, 5), (1, 0), (1, 1), (1, 2), (1, 3)]
+W1_LOADS = [(0, 4), (0, 5), (0, 2), (0, 0), (0, 3), (0, 1), (1, 4), (1, 5), (1, 2), (1, 0), (1, 3), (1, 1)]
 HEADS = rotate([("head", n, c0) for n in range(NT) for c0 in (SPLIT, 0)], 4)
 BANKS = [
     turned((0, 4), (0, 2), (0, 0), (1, 0), (2, 2)) + [("acc", THIRD, 0, 0)] + turned((3, 2)) + [("acc", THIRD, 1, 0), ("acc", LAST, 0, 2), ("acc", LAST_B, 1, 1)],
@@ -434,20 +434,20 @@ def tile_rssm_pa_kernel(tc, prev_state, prev_action, obs_bytes, obs_scale, eps,
         tensor_q = steps(turn, (0, 4), (1, 4), (0, 5), (1, 5)) + [(mm1, FRONT, 0, SL, (4,))] + steps(turn, (0, 2), (1, 2), (0, 3), (1, 3)) + [(mm1, FRONT, 0, SL, (5,))]
         tensor_q += steps(turn, (0, 0), (0, 1)) + [(mm1, FRONT, 0, SL, (2,))] + steps(turn, (1, 0), (1, 1), (2, 4), (2, 5)) + [(mm1, FRONT, 0, SL, (3, 0))]
         tensor_q += steps(turn, (2, 2), (2, 3), (2, 0), (2, 1)) + [(mm1, FRONT, 0, SL, (1,))] + steps(turn, (3, 4), (3, 5))
-        tensor_q += [(mm1, THIRD, 0, (0, 1), ALL[:2]), (mm1, FRONT, 1, SL, (4, 5)), (mm1, THIRD, 0, (0, 1), ALL[2:]), (mm1, THIRD, 0, (2, 3), ALL), (mm1, FRONT, 1, SL, (0, 2))]
+        tensor_q += [(mm1, THIRD, 0, (0, 1), ALL[:2]), (mm1, FRONT, 1, (0, 1, 2), (4,)), (mm1, THIRD, 0, (2, 3), ALL[:2]), (mm1, FRONT, 1, (3,), (4,)), (mm1, FRONT, 1, SL, (5,)), (mm1, THIRD, 0, SL, ALL[2:]), (mm1, FRONT, 1, SL, (0, 2))]
         tensor_q += steps(turn, (3, 2), (3, 3)) + [(mm1, FRONT, 1, SL, (3, 1))] + steps(turn, (3, 0), (3, 1))
         tensor_q += [(mm1, THIRD, 1, SL, ALL), (heads, 0, (0, 1)), (heads, 1, (0, 1)), (mm1, LAST, 0, (0, 1), (4, 5, 0, 1, 2, 3))]
         tensor_q += [(mm1, LAST, 0, (2, 3), ALL), (heads, 2, (0, 1)), (heads, 3, (0, 1)), (mm1, LAST_A, 1, SL, ALL), (heads, 4, (0, 1)), (heads, 5, (0, 1))]
         tensor_q += [(mm1, LAST_B, 1, SL, ALL), (heads, 6, (0, 1)), (heads, 7, (0,)), (heads, 7, (1,))]
 
         gpsimd_q = [by("gpsimd", 0, 4, 0, G0)] + [by("gpsimd", 0, g, 0, GE) for g in (5, 2)] + [by("gpsimd", 0, 3, 0, GR)]
-        gpsimd_q += [by("gpsimd", 0, 1, 0, GR), by("gpsimd", 1, 5, 0, GR), (weave_w2, 0, 0, KP, "gpsimd", 0, 64), (weave_w2, 0, KP, SPLIT, "gpsimd", 0, 32)]
+        gpsimd_q += [by("gpsimd", 0, 1, 0, GR), by("gpsimd", 1, 5), (weave_w2, 0, 0, KP, "gpsimd", 0, 64), (weave_w2, 0, KP, SPLIT, "gpsimd", 0, 32)]
         gpsimd_q += [(weave_h, THIRD, 0, "gpsimd")]
 
         scalar_q = [(widen, n, LATE, 1, "scalar") for n in (1, 2, 3)] + [by("scalar", 0, 4, G0)] + [(widen, n, LATE + 1, 1, "scalar") for n in range(4)]
         scalar_q += [(widen, n, MIXED, 1, "scalar") for n in range(4)] + [by("scalar", 0, 5, GE)] + [(widen, n, MIXED + 1, 1, "scalar") for n in range(4)]
         scalar_q += [by("scalar", 0, 2, GE), by("scalar", 0, 0), (drain, 0, 0), by("scalar", 0, 3, GR), (drain, 0, 1)] + widens(2, LATE) + steps(drain, (1, 0), (1, 1))
-        scalar_q += widens(2, MIXED) + [by("scalar", 0, 1, GR), by("scalar", 1, 4)] + widens(3, LATE) + steps(drain, (2, 0), (2, 1)) + [by("scalar", 1, 5, GR)] + relus(FRONT, 0)
+        scalar_q += widens(2, MIXED) + [by("scalar", 0, 1, GR), by("scalar", 1, 4)] + widens(3, LATE) + steps(drain, (2, 0), (2, 1)) + relus(FRONT, 0)
         scalar_q += [by("scalar", 1, 2), by("scalar", 1, 3, VR)] + relus(THIRD, 0, (0, 1)) + widens(3, MIXED) + relus(THIRD, 0, (2, 3)) + [(weave_w2, 1, 0, KP, "scalar", 0, 64), (weave_h, FRONT_A, 0, "scalar")]
         scalar_q += relus(FRONT, 1) + [(drain, 3, 0), (weave_h, FRONT_A, 1, "scalar"), (drain, 3, 1), (weave_h, FRONT_B, 0, "scalar")] + relus(THIRD, 1, (0, 1)) + [(weave_h, FRONT_B, 1, "scalar")]
 

from contextlib import ExitStack

import concourse.mybir as mybir
from concourse.masks import make_identity

B, S, A, O, H, L = 1024, 1024, 128, 1920, 1024, 384
K1 = S + A + O
FLOPS = 2 * B * K1 * H + 2 * B * H * 2 * L

F32 = mybir.dt.float32
BF16 = mybir.dt.bfloat16
U32 = mybir.dt.uint32
U8 = mybir.dt.uint8
FP8 = mybir.dt.float8_e4m3fn
FP8X4 = mybir.dt.float8_e4m3fn_x4
ACT = mybir.ActivationFunctionType
ALU = mybir.AluOpType

P = 128
KP = 4 * P
G1 = K1 // KP
G2 = H // KP
NT = B // P
QT = 2 * P
STATE_PASSES = S // KP
MIXED, LATE = STATE_PASSES, STATE_PASSES + 2
WOVEN = 4 * KP
RUNS = KP // 8
ACTION_ROWS = A // 4
SPLIT = 2 * L - KP

GROUP_TOKENS = (2 * QT, QT, QT)
FRONT, FRONT_A, FRONT_B = (0, 0, 2 * QT), (0, 0, QT), (0, QT, QT)
THIRD, LAST, LAST_A, LAST_B = (1, 0, QT), (2, 0, QT), (2, 0, P), (2, P, P)
W2_PIECES = tuple((g, c0, min(KP, 2 * L - c0)) for g in range(G2) for c0 in (0, KP))
H_PIECES = ((FRONT_A, 0), (FRONT_B, 0), (FRONT_A, 1), (FRONT_B, 1), (THIRD, 0), (THIRD, 1), (LAST, 0), (LAST_A, 1), (LAST_B, 1))
CUT = 2 * KP - A
OBS_LOADS = ((0, 1, CUT, CUT + KP), (1, 1, CUT, CUT + KP), (2, 2, CUT, CUT + KP), (0, 4, CUT + KP, O), (0, 2, 0, CUT), (2, 2, 0, CUT), (4, 2, 0, O), (6, 2, 0, O))


def rotate(keys, depth):
    return [keys[i::depth] for i in range(depth)]


def turned(*pairs):
    return [("turn",) + pair for pair in pairs]


def w(*pairs):
    return [("w",) + pair for pair in pairs]


W1_LOADS = [(0, 4), (0, 5), (0, 2), (0, 0), (0, 3), (0, 1), (1, 4), (1, 5), (1, 2), (1, 0), (1, 3), (1, 1)]
HEADS = rotate([("head", n, c0) for n in range(NT) for c0 in (SPLIT, 0)], 4)
BANKS = [
    turned((0, 4), (0, 2), (0, 0), (1, 0), (2, 2)) + [("acc", THIRD, 0, 0)] + turned((3, 2)) + [("acc", THIRD, 1, 0), ("acc", LAST, 0, 2), ("acc", LAST_B, 1, 1)],
    turned((1, 4), (1, 2), (0, 1), (1, 1), (2, 3)) + [("acc", THIRD, 0, 2)] + turned((3, 3)) + [("acc", THIRD, 1, 2), ("acc", LAST_B, 1, 2)],
    turned((0, 5), (0, 3), (2, 4), (2, 0), (3, 4), (3, 0)) + [("acc", LAST, 0, 0), ("acc", LAST_B, 1, 0)],
    turned((1, 5), (1, 3), (2, 5), (2, 1), (3, 5), (3, 1)) + [("acc", LAST_A, 1, 0), ("acc", LAST_B, 1, 3)],
] + [[("acc", FRONT, 0, t), ("acc", FRONT, 1, t)] + HEADS[t] for t in range(4)]
WOVEN_LISTS = [
    w((0, 4), (0, 5), (0, 2), (0, 3), (1, 4), (1, 5), (1, 3)) + [("w2", 0, 0)],
    w((0, 0), (1, 0)) + [("w2", 1, 0)],
    [("x", 0, 0)] + w((0, 1), (1, 2)) + [("x", 2, 2)],
    w((1, 1)) + [("w2", 1, KP)],
    [("x", 0, 4), ("x", 0, 3), ("x", 1, 2), ("x", 2, 4)],
    [("x", 0, 5), ("x", 0, 1), ("x", 2, 0), ("h", THIRD, 0)],
    [("x", 0, 2), ("x", 1, 4)],
    [("x", 1, 0)],
]
NARROW_LISTS = rotate([("w2", 0, KP), ("h", FRONT_A, 0), ("h", FRONT_A, 1), ("h", FRONT_B, 0), ("h", FRONT_B, 1),
                       ("h", THIRD, 1), ("h", LAST, 0), ("h", LAST_A, 1), ("h", LAST_B, 1)], 4)
SLICES_A_BANK = {FRONT: 1, THIRD: 2, LAST: 2, LAST_A: 4, LAST_B: 1}
PIECE = 64
G0, GE, GR, VR = 32, 44, 48, 20
BUFFERS = {
    "bank": ("psum", [P, KP], F32, BANKS),
    "obs": ("keep", [P, 2 * O], U8, [[("obs", 0, CUT), ("obs", 4, 0)], [("obs", 1, CUT), ("obs", 6, 0)]]),
    "obs_second": ("keep", [P, 2 * KP], U8, [[("obs", 2, CUT)]]),
    "obs_front": ("keep", [P, 4 * KP], U8, [[("obs", 0, CUT + KP)], [("obs", 0, 0)], [("obs", 2, 0)]]),
    "wide": ("keep", [P, 4 * KP], BF16, [[("wide", q, g), ("wide", q + 2, g)] for q in range(2) for g in (MIXED, LATE)]),
    "state": ("keep", [P, 2, S], BF16, rotate([("state", q) for q in range(4)], 2)),
    "raw": ("keep", [P, 4, KP], BF16, rotate([("raw",) + key for key in W1_LOADS], 6)),
    "raw2": ("keep", [P, 4, 2 * L], BF16, rotate([("raw2", g) for g in range(G2)], 2)),
    "woven": ("keep", [P, WOVEN], BF16, WOVEN_LISTS),
    "narrow": ("keep", [P, WOVEN // 2], BF16, NARROW_LISTS),
    "hidden": ("keep", [P, WOVEN], BF16, [[("hidden", FRONT, half)] for half in range(2)]),
    "hidden_late": ("keep", [P, WOVEN // 2], BF16, rotate([("hidden", THIRD, 0), ("hidden", THIRD, 1), ("hidden", LAST, 0),
                                                           ("hidden", LAST_A, 1)], 3)),
    "res": ("keep", [P, 2, 2 * L], F32, rotate([("res", n) for n in range(NT // 2)], 2)),
    "sample": ("keep", [P, 2, L], F32, rotate([("sample", n) for n in range(NT // 2)], 3)),
}


def tile_rssm_pa_kernel(tc, prev_state, prev_action, obs_bytes, obs_scale, eps,
                                       w1, b1, w2, b2, out_mean, out_std, out_sample):
    nc = tc.nc

    def by_tile(ap):
        return ap.rearrange("(p n) c -> p n c", n=NT)

    state_v, action_v, bytes_v, eps_v = by_tile(prev_state), by_tile(prev_action), by_tile(obs_bytes), by_tile(eps)
    mean_v, std_v, sample_v = by_tile(out_mean), by_tile(out_std), by_tile(out_sample)
    w1_v = w1.rearrange("(g p t) c -> g p t c", p=P, t=4)
    w2_v = w2.rearrange("(g p t) c -> g p t c", p=P, t=4)

    with ExitStack() as ctx:
        keep = ctx.enter_context(tc.tile_pool(name="keep", bufs=1))
        psum = ctx.enter_context(tc.psum_pool(name="psum", bufs=1))
        ctx.enter_context(tc.manual_schedule())

        w1c = keep.tile([P, G1, H], U32, align_bytes=64)
        w1s = keep.tile([P, G1, H], U8, align_bytes=64)
        w2c = keep.tile([P, G2, 2 * L], U32, align_bytes=64)
        w2s = keep.tile([P, G2, 2 * L], U8, align_bytes=64)
        xc, xs, hc, hs = [], [], [], []
        for grp, n in enumerate(GROUP_TOKENS):
            xc.append(keep.tile([P, G1, n], U32, name="xc%d" % grp, align_bytes=64))
            xs.append(keep.tile([P, G1, n], U8, name="xs%d" % grp, align_bytes=64))
            hc.append(keep.tile([P, G2, n], U32, name="hc%d" % grp, align_bytes=64))
            hs.append(keep.tile([P, G2, n], U8, name="hs%d" % grp, align_bytes=64))
        scale_mixed = keep.tile([P, 4], F32)
        scale_obs = keep.tile([P, G1 - MIXED - 1, 4], F32)
        ones = keep.tile([ACTION_ROWS, 4], F32)
        b1_cols = keep.tile([P, G2, 4], BF16)
        b2_rows = keep.tile([P, 2 * L], BF16)
        eps_sb = keep.tile([P, NT, L], BF16)
        ident = keep.tile([P, P], F32)

        tile_of, before = {}, {}
        for family, (pool_name, shape, dtype, lists) in BUFFERS.items():
            for i, keys in enumerate(lists):
                if pool_name == "psum":
                    buf = psum.tile(shape, dtype, name="%s%d" % (family, i))
                else:
                    buf = keep.tile(shape, dtype, name="%s%d" % (family, i), align_bytes=64)
                for j, key in enumerate(keys):
                    tile_of[key] = buf
                    if j:
                        before[key] = keys[j - 1]

        copy = {"vector": nc.vector.tensor_copy, "scalar": nc.scalar.copy}

        def gpsimd_copy(out, in_):
            nc.gpsimd.tensor_scalar(out=out, in0=in_, scalar1=1.0, scalar2=0.0, op0=ALU.mult, op1=ALU.add)

        def load_scales():
            flat = obs_scale.rearrange("o k -> (o k)")
            nc.sync.dma_start(out=scale_obs[:], in_=flat[KP - A:].rearrange("(g p t) -> p g t", p=P, t=4))

        def load_mixed_scales():
            mixed = obs_scale.rearrange("o k -> (o k)")[:KP - A].rearrange("(p t) -> p t", t=4)
            for p0, p1 in ((ACTION_ROWS, P // 2), (P // 2, P)):
                nc.sync.dma_start(out=scale_mixed[p0:p1, :], in_=mixed[p0 - ACTION_ROWS:p1 - ACTION_ROWS, :])

        def load_w1(half, g):
            nc.sync.dma_start(out=tile_of["raw", half, g][:], in_=w1_v[g][:, :, KP * half:KP * half + KP])

        def load_w2(g):
            nc.sync.dma_start(out=tile_of["raw2", g][:], in_=w2_v[g])

        def load_state(q):
            nc.sync.dma_start(out=tile_of["state", q][:], in_=state_v[:, 2 * q:2 * q + 2, :])

        def obs_cols(g, passes):
            return max(KP * g - S - A, 0), KP * (g + passes) - S - A

        def load_obs(n0, tiles, c0, c1):
            nc.sync.dma_start(out=tile_of["obs", n0, c0][:, :tiles * (c1 - c0)].rearrange("p (i c) -> p i c", i=tiles),
                              in_=bytes_v[:, n0:n0 + tiles, c0:c1])

        def obs_load_of(n, c0, c1):
            return [a for a in OBS_LOADS if a[0] <= n < a[0] + a[1] and a[2] <= c0 and c1 <= a[3]][0]

        def load_action(q):
            out = tile_of["wide", q, MIXED][:].rearrange("p (i c) -> p i c", i=2)[:, :, :A]
            nc.sync.dma_start(out=out, in_=action_v[:, 2 * q:2 * q + 2, :])

        def load_b1():
            nc.sync.dma_start(out=b1_cols[:], in_=b1.rearrange("(g p t) -> p g t", p=P, t=4))

        def load_b2():
            nc.sync.dma_start(out=b2_rows[:], in_=b2.partition_broadcast(P))

        def load_eps():
            nc.sync.dma_start(out=eps_sb[:], in_=eps_v)

        def widen(n, g, passes, engine):
            c0, c1 = obs_cols(g, passes)
            n0, tiles, l0, l1 = obs_load_of(n, c0, c1)
            at = (n - n0) * (l1 - l0) + c0 - l0
            end = 2 * KP * (n % 2) + KP * (g % 2 + passes)
            copy[engine](out=tile_of["wide", n // 2, g - g % 2][:, end - (c1 - c0):end],
                         in_=tile_of["obs", n0, l0][:, at:at + c1 - c0].bitcast(FP8))

        def rows(n, g):
            if g < STATE_PASSES:
                return tile_of["state", n // 2][:, n % 2, KP * g:KP * g + KP]
            at = 2 * KP * (n % 2) + KP * (g % 2)
            return tile_of["wide", n // 2, g - g % 2][:, at:at + KP]

        def turn(q, g):
            bank = tile_of["turn", q, g][:].rearrange("p (u r) -> p u r", u=2)
            for i in range(2):
                words = rows(2 * q + i, g).bitcast(F32)
                for u in range(2):
                    nc.tensor.transpose(bank[:, u, P * i:P * i + P], words[:, u::2], ident[:])

        def x_key(q, g):
            return (("x", 0, g), q) if q < 2 else (("x", q - 1, g - g % 2), g % 2)

        def x_half(q, g):
            key, j = x_key(q, g)
            return tile_of[key][:, WOVEN // 2 * j:WOVEN // 2 * (j + 1)]

        def drain(q, g):
            nc.scalar.copy(out=x_half(q, g).bitcast(F32).rearrange("p (r u) -> p r u", u=2),
                           in_=tile_of["turn", q, g][:].rearrange("p (u r) -> p r u", u=2))

        def product(q, g):
            scale = scale_mixed[:] if g == MIXED else scale_obs[:, g - MIXED - 1, :]
            nc.vector.tensor_tensor(out=x_half(q, g).rearrange("p (r u e) -> p r u e", u=2, e=2),
                                    in1=tile_of["turn", q, g][:].bitcast(BF16).rearrange("p (u r e) -> p r u e", u=2, e=2),
                                    in0=scale.rearrange("p (u e) -> p u e", e=2).unsqueeze(1).to_broadcast([P, QT, 2, 2]),
                                    op=ALU.mult)

        def quant_x(grp, g):
            n = 1 if grp == 0 else 2
            nc.vector.quantize_mx(out=xc[grp][:, g:g + n, :].rearrange("p g n -> p (g n)").bitcast(FP8X4),
                                  scales=xs[grp][:, g:g + n, :].rearrange("p g n -> p (g n)"), in_=tile_of["x", grp, g][:])

        def weave_w1(half, g, engine, r0, r1):
            woven, raw = tile_of["w", half, g][:], tile_of["raw", half, g][:]
            if engine == "gpsimd":
                gpsimd_copy(woven.rearrange("p (s m t) -> p m s t", m=P, t=4)[:, 2 * r0:2 * r1],
                            raw.rearrange("p t (m s) -> p m s t", s=4)[:, 2 * r0:2 * r1])
            else:
                copy[engine](out=woven.rearrange("p (s r e t) -> p r t e s", r=RUNS, e=2, t=4)[:, r0:r1],
                             in_=raw.rearrange("p t (r e s) -> p r t e s", e=2, s=4)[:, r0:r1])

        def quant_w1(half, g):
            cols = slice(KP * half, KP * half + KP)
            nc.vector.quantize_mx(out=w1c[:, g, cols].bitcast(FP8X4), scales=w1s[:, g, cols], in_=tile_of["w", half, g][:])

        def weave(woven, src, engine):
            if engine == "gpsimd":
                gpsimd_copy(woven.rearrange("p (c t) -> p c t", t=4), src.rearrange("p t c -> p c t"))
            else:
                copy[engine](out=woven.rearrange("p (r e t) -> p r t e", e=8, t=4),
                             in_=src.rearrange("p t (r e) -> p r t e", e=8))

        def weave_w2(g, c0, n, engine, r0, r1):
            weave(tile_of["w2", g, c0][:, 32 * r0:32 * r1], tile_of["raw2", g][:, :, c0 + 8 * r0:c0 + 8 * r1], engine)

        def quant_w2(g, c0, n):
            nc.vector.quantize_mx(out=w2c[:, g, c0:c0 + n].bitcast(FP8X4), scales=w2s[:, g, c0:c0 + n],
                                  in_=tile_of["w2", g, c0][:, :4 * n])

        def sums(span, half, t):
            n = span[2]
            first = t - t % SLICES_A_BANK[span]
            return ("acc", span, half, first), n * (t - first)

        def pairs_of(slices, passes):
            return [(t, g) for t in slices for g in passes] if len(passes) == G1 else [(t, g) for g in passes for t in slices]

        def mm1(span, half, slices, passes):
            grp, r0, n = span
            for t, g in pairs_of(slices, passes):
                key, at = sums(span, half, t)
                cols = slice(KP * half + P * t, KP * half + P * t + P)
                nc.tensor.matmul_mx(out=tile_of[key][:, at:at + n], lhsT=w1c[:, g, cols].bitcast(FP8X4), lhsT_scale=w1s[:, g, cols],
                                    rhs=xc[grp][:, g, r0:r0 + n].bitcast(FP8X4), rhs_scale=xs[grp][:, g, r0:r0 + n],
                                    start=(in_bank[key][0] == (t, g)), stop=(in_bank[key][-1] == (t, g)))

        def relu(span, half, t):
            key, at = sums(span, half, t)
            n = span[2]
            nc.scalar.activation(tile_of["hidden", span, half][:, n * t:n * t + n], tile_of[key][:, at:at + n], ACT.Relu,
                                 bias=b1_cols[:, half, t:t + 1])

        def relu_woven(span, half, t, engine):
            key, at = sums(span, half, t)
            n = span[2]
            out = tile_of["h", span, half][:, :4 * n].rearrange("p (n t) -> p n t", t=4)[:, :, t]
            if engine == "scalar":
                nc.scalar.activation(out, tile_of[key][:, at:at + n], ACT.Relu, bias=b1_cols[:, half, t:t + 1])
            else:
                nc.vector.tensor_scalar(out=out, in0=tile_of[key][:, at:at + n], scalar1=b1_cols[:, half, t:t + 1], scalar2=0.0,
                                        op0=ALU.add, op1=ALU.max)

        def parent(span):
            return FRONT if span[0] == 0 else span

        def weave_h(span, half, engine, n0=0, n1=None):
            whole = parent(span)
            src = tile_of["hidden", whole, half][:, :4 * whole[2]].rearrange("p (t n) -> p t n", t=4)
            r0, n1 = span[1] - whole[1], n1 or span[2]
            weave(tile_of["h", span, half][:, 4 * n0:4 * n1], src[:, :, r0 + n0:r0 + n1], engine)

        def quant_h(span, half):
            grp, r0, n = span
            nc.vector.quantize_mx(out=hc[grp][:, half, r0:r0 + n].bitcast(FP8X4), scales=hs[grp][:, half, r0:r0 + n],
                                  in_=tile_of["h", span, half][:, :4 * n])

        def place(n):
            grp = max(n // 2 - 1, 0)
            return grp, P * (n - (0, 4, 6)[grp])

        def heads(n, passes):
            grp, r0 = place(n)
            for c0, c1 in ((SPLIT, 2 * L), (0, SPLIT)):
                for g in passes:
                    nc.tensor.matmul_mx(out=tile_of["head", n, c0][:, :c1 - c0], lhsT=hc[grp][:, g, r0:r0 + P].bitcast(FP8X4),
                                        lhsT_scale=hs[grp][:, g, r0:r0 + P], rhs=w2c[:, g, c0:c1].bitcast(FP8X4),
                                        rhs_scale=w2s[:, g, c0:c1], start=(g == 0), stop=(g == G2 - 1))

        def res(n):
            return tile_of["res", n // 2][:, n % 2, :]

        def both(kind, n, tiles, c0, c1):
            return tile_of[kind, n // 2][:, n % 2:n % 2 + tiles, c0:c1]

        def bias(n, c0, c1):
            b0 = SPLIT * (c0 >= SPLIT)
            nc.vector.tensor_add(out=res(n)[:, c0:c1], in0=tile_of["head", n, b0][:, c0 - b0:c1 - b0], in1=b2_rows[:, c0:c1])

        def root(n, c0, c1):
            nc.scalar.activation(tile_of["sample", n // 2][:, n % 2, c0:c1], res(n)[:, L + c0:L + c1], ACT.Sqrt)

        def noise(n, tiles, c0, c1):
            part = both("sample", n, tiles, c0, c1)
            nc.vector.tensor_mul(out=part, in0=part, in1=eps_sb[:, n:n + tiles, c0:c1])

        def shift(n, tiles, c0, c1, engine):
            part = both("sample", n, tiles, c0, c1)
            add = nc.gpsimd.tensor_add if engine == "gpsimd" else nc.vector.tensor_add
            add(out=part, in0=part, in1=both("res", n, tiles, c0, c1))

        def store_std(n):
            nc.sync.dma_start(out=std_v[:, n, :], in_=res(n)[:, L:])

        def store_mean(n):
            nc.sync.dma_start(out=mean_v[:, n, :], in_=res(n)[:, :L])

        def store_sample(n, tiles, c0, c1):
            nc.sync.dma_start(out=sample_v[:, n:n + tiles, c0:c1], in_=both("sample", n, tiles, c0, c1))

        def parts(kind, n, tiles, c0, c1):
            return [(kind, n + i, c) for i in range(tiles) for c in range(c0, c1, PIECE)]

        def touches(f, *a):
            if f == load_obs:
                return [], [("obs", a[0], a[2])]
            if f == widen:
                n, g, passes = a[:3]
                load = obs_load_of(n, *obs_cols(g, passes))
                return [("obs", load[0], load[2])], [("wide", n // 2, g - g % 2)] + [("rows", n // 2, g + j) for j in range(passes)]
            if f == turn:
                q, g = a
                return [("state", q) if g < STATE_PASSES else ("rows", q, g)], [("turn", q, g)]
            if f in (drain, product):
                scales = [] if f == drain else ["mixed"] if a[1] == MIXED else ["scales"]
                return [("turn",) + a] + scales, [x_key(*a)[0]]
            if f == mm1:
                span, half, slices, passes = a
                x = [("xq", span[0], g if span[0] == 0 else g - g % 2) for g in passes]
                return x + [("wq", half, g) for g in passes], [sums(span, half, t)[0] for t in slices]
            if f == relu:
                return [sums(*a)[0], "b1"], [("hidden",) + a[:2]]
            if f == relu_woven:
                return [sums(*a[:3])[0], "b1"], [("h",) + a[:2]]
            if f == bias:
                return [("head", a[0], SPLIT * (a[1] >= SPLIT)), "b2"], [("res", a[0] // 2)] + parts("biased", a[0], 1, a[1], a[2])
            if f == root:
                return parts("biased", a[0], 1, L + a[1], L + a[2]), [("sample", a[0] // 2)] + parts("root", a[0], 1, a[1], a[2])
            if f == noise:
                return parts("root", *a) + ["eps"], parts("noise", *a)
            if f == shift:
                return parts("noise", *a[:4]) + parts("biased", *a[:4]), parts("shifted", *a[:4])
            if f in (store_std, store_mean):
                c0 = L * (f == store_std)
                return parts("biased", a[0], 1, c0, c0 + L), []
            if f == store_sample:
                return parts("shifted", *a), []
            if f == weave_h:
                return [("hidden", parent(a[0]), a[1])], [("h",) + a[:2]]
            if f == heads:
                grp, r0 = place(a[0])
                h = [("hq", span, half) for span, half in H_PIECES
                     if span[0] == grp and span[1] <= r0 < span[1] + span[2] and half in a[1]]
                return h + [("w2q",) + piece[:2] for piece in W2_PIECES], [("head", a[0], SPLIT), ("head", a[0], 0)]
            return {load_scales: ([], ["scales"]), load_mixed_scales: ([], ["mixed"]), load_b1: ([], ["b1"]),
                    load_b2: ([], ["b2"]), load_eps: ([], ["eps"]),
                    load_w1: ([], [("raw",) + a]), load_w2: ([], [("raw2",) + a]), load_state: ([], [("state",) + a]),
                    load_action: ([], [("wide",) + a + (MIXED,), ("rows",) + a + (MIXED,)]),
                    quant_x: ([("x",) + a], [("xq",) + a]),
                    weave_w1: ([("raw",) + a[:2]], [("w",) + a[:2]]), quant_w1: ([("w",) + a], [("wq",) + a]),
                    weave_w2: ([("raw2",) + a[:1]], [("w2",) + a[:2]]), quant_w2: ([("w2",) + a[:2]], [("w2q",) + a[:2]]),
                    quant_h: ([("h",) + a], [("hq",) + a])}[f]

        SL = (0, 1, 2, 3)

        def by(engine, half, g, r0=0, r1=RUNS):
            return (weave_w1, half, g, engine, r0, r1)

        def steps(f, *args):
            return [(f,) + a for a in args]

        def widens(q, g):
            return [(widen, 2 * q, g, 2, "scalar"), (widen, 2 * q + 1, g, 2, "scalar")]

        def relus(span, half, slices=SL):
            return [(relu, span, half, t) for t in slices]

        def wide(n):
            return (bias, n, SPLIT, 2 * L)

        def narrow(n):
            return (bias, n, 0, SPLIT)

        obs = [(load_obs,) + a for a in OBS_LOADS]
        w1_loads = [(load_w1,) + key for key in W1_LOADS]
        stores = []
        for n in range(NT - 2):
            stores += [(store_std, n), (store_mean, n)] + [(store_sample, n - 3, 2, 0, L)] * (n in (3, 5))
        stores += [(store_sample, 4, 1, 0, L), (store_std, 6), (store_sample, 5, 1, 0, L), (store_mean, 6), (store_std, 7), (store_mean, 7), (store_sample, 6, 1, 0, L)]
        stores += steps(store_sample, (NT - 1, 1, 0, L // 2), (NT - 1, 1, L // 2, L))
        sync_q = obs[:2] + [(load_scales,), obs[2], w1_loads[0], obs[3], w1_loads[1], obs[4], (load_action, 0), obs[5], (load_action, 1), (load_mixed_scales,)]
        sync_q += w1_loads[2:4] + [(load_state, 0), w1_loads[4], (load_state, 1), obs[6], (load_action, 2), w1_loads[5], (load_b1,)]
        sync_q += [w1_loads[6], (load_state, 2), obs[7], (load_action, 3)] + w1_loads[7:] + [(load_w2, 0), (load_w2, 1), (load_state, 3), (load_b2,), (load_eps,)] + stores

        ALL = (4, 5, 2, 3, 0, 1)
        tensor_q = steps(turn, (0, 4), (1, 4), (0, 5), (1, 5)) + [(mm1, FRONT, 0, SL, (4,))] + steps(turn, (0, 2), (1, 2), (0, 3), (1, 3)) + [(mm1, FRONT, 0, SL, (5,))]
        tensor_q += steps(turn, (0, 0), (0, 1)) + [(mm1, FRONT, 0, SL, (2,))] + steps(turn, (1, 0), (1, 1), (2, 4), (2, 5)) + [(mm1, FRONT, 0, SL, (3, 0))]
        tensor_q += steps(turn, (2, 2), (2, 3), (2, 0), (2, 1)) + [(mm1, FRONT, 0, SL, (1,))] + steps(turn, (3, 4), (3, 5))
        tensor_q += [(mm1, THIRD, 0, (0, 1), ALL[:2]), (mm1, FRONT, 1, (0, 1, 2), (4,)), (mm1, THIRD, 0, (2, 3), ALL[:2]), (mm1, FRONT, 1, (3,), (4,)), (mm1, FRONT, 1, SL, (5,)), (mm1, THIRD, 0, SL, ALL[2:]), (mm1, FRONT, 1, SL, (0, 2))]
        tensor_q += steps(turn, (3, 2), (3, 3)) + [(mm1, FRONT, 1, SL, (3, 1))] + steps(turn, (3, 0), (3, 1))
        tensor_q += [(mm1, THIRD, 1, SL, ALL), (heads, 0, (0, 1)), (heads, 1, (0, 1)), (mm1, LAST, 0, (0, 1), (4, 5, 0, 1, 2, 3))]
        tensor_q += [(mm1, LAST, 0, (2, 3), ALL), (heads, 2, (0, 1)), (heads, 3, (0, 1)), (mm1, LAST_A, 1, SL, ALL), (heads, 4, (0, 1)), (heads, 5, (0, 1))]
        tensor_q += [(mm1, LAST_B, 1, SL, ALL), (heads, 6, (0, 1)), (heads, 7, (0,)), (heads, 7, (1,))]

        gpsimd_q = [by("gpsimd", 0, 4, 0, G0)] + [by("gpsimd", 0, g, 0, GE) for g in (5, 2)] + [by("gpsimd", 0, 3, 0, GR)]
        gpsimd_q += [by("gpsimd", 0, 1, 0, GR), by("gpsimd", 1, 5), (weave_w2, 0, 0, KP, "gpsimd", 0, 64), (weave_w2, 0, KP, SPLIT, "gpsimd", 0, 32)]
        gpsimd_q += [(weave_h, THIRD, 0, "gpsimd")]

        scalar_q = [(widen, n, LATE, 1, "scalar") for n in (1, 2, 3)] + [by("scalar", 0, 4, G0)] + [(widen, n, LATE + 1, 1, "scalar") for n in range(4)]
        scalar_q += [(widen, n, MIXED, 1, "scalar") for n in range(4)] + [by("scalar", 0, 5, GE)] + [(widen, n, MIXED + 1, 1, "scalar") for n in range(4)]
        scalar_q += [by("scalar", 0, 2, GE), by("scalar", 0, 0), (drain, 0, 0), by("scalar", 0, 3, GR), (drain, 0, 1)] + widens(2, LATE) + steps(drain, (1, 0), (1, 1))
        scalar_q += widens(2, MIXED) + [by("scalar", 0, 1, GR), by("scalar", 1, 4)] + widens(3, LATE) + steps(drain, (2, 0), (2, 1)) + relus(FRONT, 0)
        scalar_q += [by("scalar", 1, 2), by("scalar", 1, 3, VR)] + relus(THIRD, 0, (0, 1)) + widens(3, MIXED) + relus(THIRD, 0, (2, 3)) + [(weave_w2, 1, 0, KP, "scalar", 0, 64), (weave_h, FRONT_A, 0, "scalar")]
        scalar_q += relus(FRONT, 1) + [(drain, 3, 0), (weave_h, FRONT_A, 1, "scalar"), (drain, 3, 1), (weave_h, FRONT_B, 0, "scalar")] + relus(THIRD, 1, (0, 1)) + [(weave_h, FRONT_B, 1, "scalar")]

        vector_q = [(widen, 0, LATE, 1, "vector")] + steps(product, (0, 4), (1, 4)) + [(quant_w1, 0, 4), (quant_x, 0, 4)]
        vector_q += steps(product, (0, 5), (1, 5)) + [(quant_w1, 0, 5), (quant_x, 0, 5)] + steps(product, (0, 2), (1, 2))
        vector_q += [(quant_w1, 0, 2), (quant_x, 0, 2)] + steps(product, (0, 3), (1, 3)) + [(quant_w1, 0, 3), (quant_x, 0, 3), (quant_x, 0, 0), (quant_w1, 0, 0)]
        vector_q += steps(product, (2, 4), (2, 5)) + [(quant_x, 0, 1), (quant_w1, 0, 1), (quant_w1, 1, 4), (quant_x, 1, 4)] + steps(product, (2, 2), (2, 3))
        vector_q += [(quant_w1, 1, 5), (quant_x, 1, 2), (quant_x, 1, 0), by("vector", 1, 0), by("vector", 1, 3, 0, VR), (quant_w1, 1, 0), (quant_w1, 1, 2), by("vector", 1, 1), (quant_w1, 1, 3), (quant_w1, 1, 1)]
        vector_q += steps(product, (3, 4), (3, 5), (3, 2), (3, 3))
        vector_q += [(quant_w2, 0, 0, KP), (quant_w2, 1, 0, KP), (weave_w2, 1, KP, SPLIT, "vector", 0, 32), (quant_w2, 0, KP, SPLIT), (quant_h, FRONT_A, 0), (quant_w2, 1, KP, SPLIT), (quant_h, FRONT_A, 1), (quant_x, 2, 4), (quant_x, 2, 0), (quant_x, 2, 2)]

        def sample(n):
            return [(noise, n, 1, 0, L), (shift, n, 1, 0, L, "vector")]

        def rooted(n):
            return (root, n, 0, L)

        end, mid = NT - 1, L // 2
        scalar_q += [rooted(0)] + relus(THIRD, 1, (2, 3)) + [rooted(1), (weave_h, THIRD, 1, "scalar")] + relus(LAST, 0) + [rooted(2)]
        scalar_q += [(weave_h, LAST, 0, "scalar", 0, P), rooted(3), (weave_h, LAST, 0, "scalar", P)] + relus(LAST_A, 1) + [(weave_h, LAST_A, 1, "scalar"), rooted(4)]
        scalar_q += [(relu_woven, LAST_B, 1, t, "scalar") for t in SL[:1]] + [rooted(5)] + [(relu_woven, LAST_B, 1, t, "scalar") for t in SL[1:]] + [rooted(6), (root, end, 0, mid), (root, end, mid, L)]
        vector_q += [wide(0), wide(1), narrow(0), narrow(1), (quant_h, FRONT_B, 0), (quant_h, FRONT_B, 1), sample(0)[0], (quant_h, THIRD, 0), sample(1)[0], sample(0)[1], sample(1)[1]]
        vector_q += [wide(2), narrow(2), wide(3), narrow(3), (quant_h, THIRD, 1), sample(2)[0], sample(3)[0], sample(2)[1], wide(4), sample(3)[1], narrow(4), wide(5), narrow(5)]
        vector_q += [(quant_h, LAST, 0), (quant_h, LAST_A, 1), sample(4)[0], sample(5)[0], sample(4)[1], wide(6), (quant_h, LAST_B, 1), sample(5)[1], narrow(6)]
        vector_q += [(bias, end, L, L + mid), (bias, end, L + mid, 2 * L), sample(6)[0], narrow(end), (bias, end, SPLIT, L), sample(6)[1]]
        vector_q += [(noise, end, 1, 0, mid), (noise, end, 1, mid, L), (shift, end, 1, 0, mid, "vector"), (shift, end, 1, mid, L, "vector")]

        in_bank = {}
        for step in tensor_q:
            if step[0] == mm1:
                for t, g in pairs_of(*step[3:]):
                    in_bank.setdefault(sums(step[1], step[2], t)[0], []).append((t, g))

        nc.vector.memset(ones[:], 1.0)
        make_identity(nc, ident[:])
        nc.scalar.activation(scale_mixed[:ACTION_ROWS, :], ones[:], ACT.Sqrt)

        queues = [sync_q, tensor_q, scalar_q, vector_q, gpsimd_q]
        def holder(key):
            part_of = {"biased": "res", "root": "sample", "noise": "sample", "shifted": "sample"}
            if key[0] == "rows":
                return ("wide", key[1], key[2] - key[2] % 2)
            return (part_of[key[0]], key[1] // 2) if key[0] in part_of else key

        writers, users = {}, {}
        for step in [step for queue in queues for step in queue]:
            reads, writes = touches(*step)
            for key in writes:
                writers.setdefault(key, []).append(step)
            for key in reads + writes:
                users.setdefault(holder(key), []).append(step)
        done = set()
        while any(queues):
            moved = False
            for queue in queues:
                if not queue:
                    continue
                reads, writes = touches(*queue[0])
                waits = [s for key in reads for s in writers.get(key, [])]
                waits += [s for key in writes if key in before for s in users[before[key]]]
                if all(s in done for s in waits):
                    step = queue.pop(0)
                    step[0](*step[1:])
                    done.add(step)
                    moved = True
            assert moved
